import numpy as np
import ml_dtypes


def mxq(x, axis, fmt="e4m3"):
    dtype, down = {"e4m3": (ml_dtypes.float8_e4m3fn, 7), "e5m2": (ml_dtypes.float8_e5m2, 14)}[fmt]
    v = np.moveaxis(np.asarray(x, np.float32).astype(ml_dtypes.bfloat16).astype(np.float64), axis, -1)
    blocks = v.reshape(v.shape[:-1] + (-1, 32))
    amax = np.abs(blocks).max(-1, keepdims=True)
    byte = np.maximum(np.where(amax > 0, np.frexp(amax)[1] - 1 + 127, 0) - down, 1)
    scale = np.exp2(byte - 127.0)
    codes = (blocks / scale).astype(np.float32).astype(dtype).astype(np.float64)
    return np.moveaxis((codes * scale).reshape(v.shape), -1, axis)


WIDE = False


def mx_kscale(k):
    if not WIDE:
        return np.ones(k)
    levels = np.array([10, -10, 5, -5, 0])
    if k % 512:
        return np.exp2(np.random.permutation(np.resize(levels, k // 32))).repeat(32)
    a = np.empty((k // 512, 16))
    for p in range(k // 512):
        a[p, :8] = np.random.permutation(np.resize(levels, 8))
        for g in range(8):
            far = levels[np.abs(levels - a[p, g]) >= 10]
            a[p, g + 8] = far[np.random.randint(len(far))]
    return np.exp2(a.ravel()).repeat(32)


BF16 = ml_dtypes.bfloat16


def bf(x):
    return np.asarray(x, np.float32).astype(BF16)


def f64(x):
    return np.asarray(x).astype(np.float64)


B, N, R, DE, DR, NUM_BASES, OUT_DIM = 1, 1024, 16, 128, 64, 256, 128
F = DE + DR
KS = R * F


def draw0():
    s = mx_kscale(N)
    t = mx_kscale(KS)[:F]
    deg = np.random.uniform(0.5, 1.5, (B, R, N, 1))
    adj = np.random.uniform(0.0, 1.0, (B, R, N, N)) * deg / np.sqrt(N)
    return {"node_features": bf(np.random.standard_normal((B, N, DE)) * 2.0 / s[:, None] * t[:DE]),
            "relation_features": bf(np.random.standard_normal((B, R, DR)) * 2.0 / np.sqrt(N) / s.mean() * t[DE:]),
            "adj": bf(adj * s),
            "Wb": bf(np.random.standard_normal((NUM_BASES, KS)) / np.sqrt(KS) / np.tile(t, R))}


def core(node_features, relation_features, adj, Wb):
    a = f64(adj)
    node_part = mxq(a, 3, "e4m3") @ mxq(f64(node_features), 1, "e4m3")[:, None]
    row_sum = a.sum(-1)
    rel_part = row_sum[..., None] * f64(relation_features)[:, :, None, :]
    supports = np.concatenate([node_part, rel_part], -1)
    supports = supports.transpose(0, 2, 1, 3).reshape(B, N, KS)
    return mxq(supports, 2, "e4m3") @ mxq(f64(Wb), 1, "e4m3").T


def e4m3fn_bytes(y):
    return np.clip(np.asarray(y, np.float64), -448.0, 448.0).astype(np.float32).astype(ml_dtypes.float8_e4m3fn).view(np.uint8)


def e4m3fn_values(b):
    return np.asarray(b, np.uint8).view(ml_dtypes.float8_e4m3fn).astype(np.float64)


def setup_inputs():
    d = draw0()
    x0 = np.asarray(d['Wb']).astype(np.float64)
    s = (np.max(np.abs(x0), axis=(0,), keepdims=True) / 448.0).astype(np.float32)
    out = {}
    for k, v in d.items():
        if k == 'Wb':
            out['Wb_bytes'] = e4m3fn_bytes(x0 / s.astype(np.float64))
            out['Wb_scale'] = s
        else:
            out[k] = v
    return out


def reference(node_features, relation_features, adj, Wb_bytes, Wb_scale):
    return core(node_features, relation_features, adj, e4m3fn_values(Wb_bytes) * Wb_scale.astype(np.float64))

@@ -1,0 +1,387 @@
+from contextlib import ExitStack
+
+import concourse.mybir as mybir
+from concourse.masks import make_identity
+
+N = 1024
+R = 16
+DE = 128
+DR = 64
+F = DE + DR
+NB = 256
+P = 128
+IT = N // P
+RG = 4
+GROUPS = R // RG
+STEPS = IT * GROUPS
+PREFETCH = 5
+SCALAR_SUMS = (3, 5, 7, 9, 10, 11, 12, 13, 14, 15, 16, 19, 23, 25, 27)
+
+F32 = mybir.dt.float32
+BF16 = mybir.dt.bfloat16
+U32 = mybir.dt.uint32
+U8 = mybir.dt.uint8
+FP8 = mybir.dt.float8_e4m3fn
+FP8X4 = mybir.dt.float8_e4m3fn_x4
+MULT = mybir.AluOpType.mult
+ADD = mybir.AluOpType.add
+
+FLOPS = 2 * (R * N * N * DE + N * R * F * NB)
+
+
+def tile_relationalgraphconvolution_pa_kernel(
+    tc, node_features, relation_features, adj, Wb_bytes, Wb_scale, out
+):
+    nc = tc.nc
+    with ExitStack() as ctx:
+        keep = ctx.enter_context(tc.tile_pool(name="keep", bufs=1))
+        rawp = ctx.enter_context(tc.tile_pool(name="rawp", bufs=PREFETCH + 1))
+        work = ctx.enter_context(tc.tile_pool(name="work", bufs=2))
+        three = ctx.enter_context(tc.tile_pool(name="three", bufs=3))
+        late = ctx.enter_context(tc.tile_pool(name="late", bufs=6))
+        xtp = ctx.enter_context(tc.psum_pool(name="xtp", bufs=5))
+        mxp = ctx.enter_context(tc.psum_pool(name="mxp", bufs=2))
+        outp = ctx.enter_context(tc.psum_pool(name="outp", bufs=1))
+        ctx.enter_context(tc.manual_schedule())
+
+        ident = keep.tile([P, P], F32, name="ident", align_bytes=64)
+        make_identity(nc, ident[:])
+        select = keep.tile([P, 4, P], BF16, name="select", align_bytes=64)
+        nc.vector.memset(select[:], 0.0)
+        for u in range(2):
+            for h in range(2):
+                nc.vector.tensor_copy(
+                    out=select[:, 2 * u + h, :].rearrange("p (b x h) -> p b x h", x=4, h=2)[:, :, :, h],
+                    in_=ident[:].rearrange("p (b u x) -> p b u x", u=2, x=4)[:, :, u, :],
+                )
+        nf_raw = keep.tile([P, 2, 4, DE], BF16, name="nf_raw", align_bytes=64)
+        nf_grp = keep.tile([P, 2, DE, 4], BF16, name="nf_grp", align_bytes=64)
+        nf_codes = keep.tile([P, 2 * DE], U32, name="nf_codes", align_bytes=64)
+        nf_scales = keep.tile([P, 2 * DE], U8, name="nf_scales", align_bytes=64)
+        relf = keep.tile([P, R * DR], BF16, name="relf", align_bytes=64)
+        w_bytes = keep.tile([P, 2 * R * F], U8, name="w_bytes", align_bytes=64)
+        w_scale = keep.tile([P, R * F], F32, name="w_scale", align_bytes=64)
+        w_val = keep.tile([P, 2 * R * F], BF16, name="w_val", align_bytes=64)
+        w_grp = keep.tile([P, 6 * NB * 4], BF16, name="w_grp", align_bytes=64)
+        w_codes = keep.tile([P, 6 * NB], U32, name="w_codes", align_bytes=64)
+        w_scales = keep.tile([P, 6 * NB], U8, name="w_scales", align_bytes=64)
+
+        raw = {}
+        perm = {}
+        grp = {}
+        codes = {}
+        scales = {}
+        mx = {}
+        rs = {}
+        supn = {}
+        supr = {}
+        sgrp = {}
+        scodes = {}
+        sscales = {}
+        obank = {}
+
+        def load(s, pieces=1):
+            it, g = s // GROUPS, s % GROUPS
+            raw[s] = rawp.tile([P, RG, N], BF16, name="raw", align_bytes=64)
+            n = RG // pieces
+            for a in range(pieces):
+                r0 = g * RG + a * n
+                nc.sync.dma_start(
+                    out=raw[s][:, a * n : (a + 1) * n, :],
+                    in_=adj[0, r0 : r0 + n, it * P : (it + 1) * P, :].rearrange("r i j -> i r j"),
+                )
+
+        def load_weight_bytes(h, f0, width):
+            c0 = h * R * F + f0 * R
+            rows = Wb_bytes[h * P : (h + 1) * P, :].rearrange("n (r f) -> n r f", f=F)
+            nc.sync.dma_start(
+                out=w_bytes[:, c0 : c0 + R * width].rearrange("p (r d) -> p r d", d=width),
+                in_=rows[:, :, f0 : f0 + width],
+            )
+
+        def load_weight_scale(f0, width):
+            sc = Wb_scale.rearrange("o (r f) -> (o r) f", f=F)
+            nc.sync.dma_start(
+                out=w_scale[:, f0 * R : f0 * R + R * width].rearrange("p (r d) -> p r d", d=width),
+                in_=sc[:, f0 : f0 + width].partition_broadcast(P),
+            )
+
+        def open_step(s):
+            it, g = s // GROUPS, s % GROUPS
+            if g == 0:
+                rs[it] = late.tile([P, R], F32, name="rs")
+                supn[it] = three.tile([P, R * DE], BF16, name="supn", align_bytes=64)
+                supr[it] = three.tile([P, R * DR], BF16, name="supr", align_bytes=64)
+            perm[s] = three.tile([P, RG * N], BF16, name="perm", align_bytes=64)
+
+        def reorder(s, a):
+            it, g = s // GROUPS, s % GROUPS
+            r = g * RG + a
+            dst = perm[s][:, a * N : (a + 1) * N].rearrange("p (u q f) -> p u q f", u=2, f=16)
+            src = raw[s][:, a, :].rearrange("p (q u f) -> p u q f", u=2, f=16)
+            if a == RG - 1 and s in SCALAR_SUMS:
+                nc.scalar.activation(
+                    out=dst,
+                    in_=src,
+                    func=mybir.ActivationFunctionType.Copy,
+                    accum_out=rs[it][:, r : r + 1],
+                )
+            else:
+                nc.vector.tensor_scalar(
+                    out=dst,
+                    in0=src,
+                    scalar1=1.0,
+                    scalar2=None,
+                    op0=MULT,
+                    op1=ADD,
+                    accum_out=rs[it][:, r : r + 1],
+                )
+
+        def relation_part(s, a, n):
+            it, g = s // GROUPS, s % GROUPS
+            r0 = g * RG + a
+            cols = slice(r0 * DR, (r0 + n) * DR)
+            nc.gpsimd.tensor_tensor(
+                out=supr[it][:, cols].rearrange("p (r d) -> p r d", d=DR),
+                in0=relf[:, cols].rearrange("p (r d) -> p r d", d=DR),
+                in1=rs[it][:, r0 : r0 + n].unsqueeze(2).to_broadcast([P, n, DR]),
+                op=MULT,
+            )
+
+        def turn(s):
+            grp[s] = three.tile([P, RG * N], BF16, name="grp", align_bytes=64)
+            for a in range(RG):
+                bank = xtp.tile([P, 512], F32, name="xt")
+                for c in range(2):
+                    for u in range(2):
+                        k0 = (c * 2 + u) * P
+                        w0 = a * 512 + u * 256 + c * P
+                        nc.tensor.transpose(bank[:, k0 : k0 + P], perm[s][:].bitcast(F32)[:, w0 : w0 + P], ident[:])
+                nc.scalar.copy(
+                    out=grp[s][:, a * N : (a + 1) * N].bitcast(F32).rearrange("p (c i u) -> p c i u", c=2, u=2),
+                    in_=bank[:].rearrange("p (c u i) -> p c i u", c=2, u=2),
+                )
+
+        def quantise(s, a0=0, n=RG):
+            if a0 == 0:
+                codes[s] = three.tile([P, N], U32, name="codes", align_bytes=64)
+                scales[s] = three.tile([P, N], U8, name="scales", align_bytes=64)
+            cols = slice(a0 * 256, (a0 + n) * 256)
+            nc.vector.quantize_mx(
+                out=codes[s][:, cols].bitcast(FP8X4),
+                scales=scales[s][:, cols],
+                in_=grp[s][:, a0 * N : (a0 + n) * N],
+            )
+
+        def aggregate(s, a0=0, n=RG):
+            if a0 == 0:
+                mx[s] = mxp.tile([P, RG * DE], F32, name="mx")
+            for a in range(a0, a0 + n):
+                for c in range(2):
+                    cols = slice(a * 256 + c * P, a * 256 + (c + 1) * P)
+                    nf_cols = slice(c * DE, (c + 1) * DE)
+                    nc.tensor.matmul_mx(
+                        out=mx[s][:, a * DE : (a + 1) * DE],
+                        lhsT=codes[s][:, cols].bitcast(FP8X4),
+                        lhsT_scale=scales[s][:, cols],
+                        rhs=nf_codes[:, nf_cols].bitcast(FP8X4),
+                        rhs_scale=nf_scales[:, nf_cols],
+                        start=(c == 0),
+                        stop=(c == 1),
+                    )
+
+        def keep_supports(s, a0=0, n=RG):
+            it, g = s // GROUPS, s % GROUPS
+            dst = supn[it][:, g * 512 : (g + 1) * 512].rearrange("p (u q e) -> p u q e", u=2, e=2)
+            nc.scalar.copy(
+                out=dst[:, :, a0 * 32 : (a0 + n) * 32, :],
+                in_=mx[s][:, a0 * DE : (a0 + n) * DE].rearrange("p (q u e) -> p u q e", u=2, e=2),
+            )
+
+        def turn_supports(it, q0, n, copy=nc.scalar.copy):
+            if q0 == 0:
+                sgrp[it] = work.tile([P, 6 * 512], BF16, name="sgrp", align_bytes=64)
+            bank = xtp.tile([P, 512], F32, name="xt")
+            for b in range(n):
+                for u in range(2):
+                    k0 = (b * 2 + u) * P
+                    q = q0 + b
+                    if q < 4:
+                        w0 = q * 256 + u * P
+                        src = supn[it][:].bitcast(F32)[:, w0 : w0 + P]
+                    else:
+                        w0 = (q - 4) * 256
+                        src = supr[it][:].bitcast(F32)[:, w0 + u : w0 + 256 : 2]
+                    nc.tensor.transpose(bank[:, k0 : k0 + P], src, ident[:])
+            copy(
+                out=sgrp[it][:, q0 * 512 : (q0 + n) * 512]
+                .bitcast(F32)
+                .rearrange("p (b i u) -> p b i u", b=n, u=2),
+                in_=bank[:, 0 : n * 256].rearrange("p (b u i) -> p b i u", b=n, u=2),
+            )
+
+        def quantise_supports(it, q0, n):
+            if q0 == 0:
+                scodes[it] = late.tile([P, 6 * P], U32, name="scodes", align_bytes=64)
+                sscales[it] = late.tile([P, 6 * P], U8, name="sscales", align_bytes=64)
+            cols = slice(q0 * P, (q0 + n) * P)
+            nc.vector.quantize_mx(
+                out=scodes[it][:, cols].bitcast(FP8X4),
+                scales=sscales[it][:, cols],
+                in_=sgrp[it][:, q0 * 512 : (q0 + n) * 512],
+            )
+
+        def project(it, passes, first, last):
+            if first:
+                obank[it] = outp.tile([P, NB], F32, name="o")
+            for j, q in enumerate(passes):
+                cols = slice(q * P, (q + 1) * P)
+                w_cols = slice(q * NB, (q + 1) * NB)
+                nc.tensor.matmul_mx(
+                    out=obank[it][:],
+                    lhsT=scodes[it][:, cols].bitcast(FP8X4),
+                    lhsT_scale=sscales[it][:, cols],
+                    rhs=w_codes[:, w_cols].bitcast(FP8X4),
+                    rhs_scale=w_scales[:, w_cols],
+                    start=(first and j == 0),
+                    stop=(last and j == len(passes) - 1),
+                )
+
+        def store(it):
+            res = work.tile([P, NB], F32, name="res", align_bytes=64)
+            nc.scalar.copy(out=res[:], in_=obank[it][:])
+            nc.sync.dma_start(out=out[0, it * P : (it + 1) * P, :], in_=res[:])
+
+        def weight_values(h, pair):
+            c0 = h * R * F + pair * 1024
+            nc.vector.tensor_tensor(
+                out=w_val[:, c0 : c0 + 1024],
+                in0=w_bytes[:, c0 : c0 + 1024].bitcast(FP8),
+                in1=w_scale[:, pair * 1024 : (pair + 1) * 1024],
+                op=MULT,
+            )
+
+        def turn_weights(q):
+            bank = xtp.tile([P, 512], F32, name="xt")
+            words = w_val[:].bitcast(F32)
+            for h in range(2):
+                for u in range(2):
+                    k0 = (h * 2 + u) * P
+                    w0 = h * (R * F // 2) + q * 256
+                    nc.tensor.transpose(bank[:, k0 : k0 + P], words[:, w0 + u : w0 + 256 : 2], ident[:])
+            nc.scalar.copy(
+                out=w_grp[:, q * 1024 : (q + 1) * 1024].bitcast(F32).rearrange("p (h n u) -> p h n u", h=2, u=2),
+                in_=bank[:].rearrange("p (h u n) -> p h n u", h=2, u=2),
+            )
+
+        def quantise_weights(pair):
+            cols = slice(pair * 512, (pair + 1) * 512)
+            nc.vector.quantize_mx(
+                out=w_codes[:, cols].bitcast(FP8X4),
+                scales=w_scales[:, cols],
+                in_=w_grp[:, pair * 2048 : (pair + 1) * 2048],
+            )
+
+        load(0, 4)
+        nc.sync.dma_start(
+            out=nf_raw[:], in_=node_features[0].rearrange("(c p t) d -> p c t d", p=P, t=4)
+        )
+        load(1, 2)
+        nc.sync.dma_start(
+            out=relf[:], in_=relation_features[0].rearrange("r d -> (r d)").partition_broadcast(P)
+        )
+        for s in range(2, PREFETCH):
+            load(s)
+
+        open_step(0)
+        for a in range(RG):
+            reorder(0, a)
+        relation_part(0, 0, RG)
+        for c in range(2):
+            bank = xtp.tile([P, 512], F32, name="xt")
+            for u in range(2):
+                for h in range(2):
+                    nc.tensor.matmul(
+                        bank[:, u * 256 : (u + 1) * 256],
+                        lhsT=select[:, 2 * u + h, :],
+                        rhs=nf_raw[:, c, 2 * h : 2 * h + 2, :].rearrange("p e d -> p (e d)"),
+                        start=(h == 0),
+                        stop=(h == 1),
+                    )
+            nc.scalar.copy(out=nf_grp[:, c], in_=bank[:].rearrange("p (t d) -> p d t", t=4))
+        nc.vector.quantize_mx(
+            out=nf_codes[:].bitcast(FP8X4),
+            scales=nf_scales[:],
+            in_=nf_grp[:].rearrange("p c d t -> p (c d t)"),
+        )
+
+        project_at = {}
+        for it in range(IT - 1):
+            project_at[max(4 * it + 8, 21 + it)] = it
+        weight_loads = {
+            2: (load_weight_bytes, (0, 0, DE)),
+            3: (load_weight_bytes, (0, DE, DR)),
+            4: (load_weight_bytes, (1, 0, DE)),
+            5: (load_weight_bytes, (1, DE, DR)),
+            6: (load_weight_scale, (0, DE)),
+            8: (load_weight_scale, (DE, DR)),
+        }
+
+        for s in range(STEPS):
+            if s + PREFETCH < STEPS:
+                load(s + PREFETCH)
+            if s in weight_loads:
+                fn, args = weight_loads[s]
+                fn(*args)
+            if s + 1 < STEPS:
+                open_step(s + 1)
+                reorder(s + 1, 0)
+            if s >= 1:
+                quantise(s - 1)
+            turn(s)
+            for q0, at in ((0, 4), (4, 5), (2, 6)):
+                if s >= at and (s - at) % 4 == 0:
+                    turn_supports((s - at) // 4, q0, 2)
+            if 16 <= s < 19:
+                turn_weights(2 * (s - 16))
+                turn_weights(2 * (s - 16) + 1)
+            if s >= 2:
+                aggregate(s - 2)
+                keep_supports(s - 2)
+            if 10 <= s < 16:
+                weight_values((s - 10) % 2, (s - 10) // 2)
+            if 17 <= s < 20:
+                quantise_weights(s - 17)
+            for q0, at in ((0, 5), (4, 6), (2, 7)):
+                if s >= at and (s - at) % 4 == 0:
+                    quantise_supports((s - at) // 4, q0, 2)
+            if s + 1 < STEPS:
+                reorder(s + 1, 1)
+                relation_part(s + 1, 0, 2)
+                reorder(s + 1, 2)
+                reorder(s + 1, 3)
+                relation_part(s + 1, 2, 2)
+            if s in project_at:
+                project(project_at[s], range(6), True, True)
+                store(project_at[s])
+
+        it, s = IT - 1, STEPS - 1
+        project(it - 1, range(6), True, True)
+        store(it - 1)
+        aggregate(s - 1)
+        keep_supports(s - 1)
+        for a in range(RG):
+            quantise(s, a, 1)
+        turn_supports(it, 0, 2, nc.vector.tensor_copy)
+        turn_supports(it, 4, 2, nc.vector.tensor_copy)
+        aggregate(s)
+        keep_supports(s)
+        turn_supports(it, 2, 1, nc.vector.tensor_copy)
+        quantise_supports(it, 0, 2)
+        quantise_supports(it, 4, 2)
+        quantise_supports(it, 2, 1)
+        project(it, (0, 1, 4, 5, 2), True, False)
+        turn_supports(it, 3, 1)
+        quantise_supports(it, 3, 1)
+        project(it, (3,), False, True)
+        store(it)

@@ -14,8 +14,13 @@ IT = N // P
 RG = 4
 GROUPS = R // RG
 STEPS = IT * GROUPS
+HALVES = STEPS // 2
 PREFETCH = 5
-SCALAR_SUMS = (3, 5, 7, 9, 10, 11, 12, 13, 14, 15, 16, 19, 23, 25, 27)
+TENSOR_A = 1
+W0 = 4
+VECTOR_EXITS = 61
+FIRST_PROJECT = 12
+SCALAR_STEPS = tuple(range(4, 12)) + tuple(range(12, 26, 2))
 
 F32 = mybir.dt.float32
 BF16 = mybir.dt.bfloat16
@@ -29,6 +34,14 @@ ADD = mybir.AluOpType.add
 FLOPS = 2 * (R * N * N * DE + N * R * F * NB)
 
 
+def on_tensor(s, a):
+    return a == TENSOR_A and s % 2 == 1 and s < STEPS - 1
+
+
+def on_scalar(s, a):
+    return a == 0 and s in SCALAR_STEPS
+
+
 def tile_relationalgraphconvolution_pa_kernel(
     tc, node_features, relation_features, adj, Wb_bytes, Wb_scale, out
 ):
@@ -36,29 +49,29 @@ def tile_relationalgraphconvolution_pa_kernel(
     with ExitStack() as ctx:
         keep = ctx.enter_context(tc.tile_pool(name="keep", bufs=1))
         rawp = ctx.enter_context(tc.tile_pool(name="rawp", bufs=PREFETCH + 1))
+        permp = ctx.enter_context(tc.tile_pool(name="permp", bufs=12))
         work = ctx.enter_context(tc.tile_pool(name="work", bufs=2))
         three = ctx.enter_context(tc.tile_pool(name="three", bufs=3))
         late = ctx.enter_context(tc.tile_pool(name="late", bufs=6))
-        xtp = ctx.enter_context(tc.psum_pool(name="xtp", bufs=5))
+        xtp = ctx.enter_context(tc.psum_pool(name="xtp", bufs=4))
         mxp = ctx.enter_context(tc.psum_pool(name="mxp", bufs=2))
         outp = ctx.enter_context(tc.psum_pool(name="outp", bufs=1))
+        sump = ctx.enter_context(tc.psum_pool(name="sump", bufs=1))
         ctx.enter_context(tc.manual_schedule())
 
         ident = keep.tile([P, P], F32, name="ident", align_bytes=64)
         make_identity(nc, ident[:])
-        select = keep.tile([P, 4, P], BF16, name="select", align_bytes=64)
-        nc.vector.memset(select[:], 0.0)
-        for u in range(2):
-            for h in range(2):
-                nc.vector.tensor_copy(
-                    out=select[:, 2 * u + h, :].rearrange("p (b x h) -> p b x h", x=4, h=2)[:, :, :, h],
-                    in_=ident[:].rearrange("p (b u x) -> p b u x", u=2, x=4)[:, :, u, :],
-                )
-        nf_raw = keep.tile([P, 2, 4, DE], BF16, name="nf_raw", align_bytes=64)
-        nf_grp = keep.tile([P, 2, DE, 4], BF16, name="nf_grp", align_bytes=64)
-        nf_codes = keep.tile([P, 2 * DE], U32, name="nf_codes", align_bytes=64)
-        nf_scales = keep.tile([P, 2 * DE], U8, name="nf_scales", align_bytes=64)
-        relf = keep.tile([P, R * DR], BF16, name="relf", align_bytes=64)
+        rs = keep.tile([P, IT * R], F32, name="rs", align_bytes=64)
+        nc.vector.memset(rs[:], 0.0)
+        mask = keep.tile([P, P], BF16, name="mask", align_bytes=64)
+        m0 = (RG + TENSOR_A) * 16
+        nc.vector.memset(mask[:], 0.0)
+        nc.vector.memset(mask[:, m0 : m0 + 16], 1.0)
+        nf_raw = keep.tile([P, 4, 4 * DE], BF16, name="nf_raw", align_bytes=64)
+        nf_grp = keep.tile([P, 4 * 4 * DE], BF16, name="nf_grp", align_bytes=64)
+        nf_codes = keep.tile([P, 4 * DE], U32, name="nf_codes", align_bytes=64)
+        nf_scales = keep.tile([P, 4 * DE], U8, name="nf_scales", align_bytes=64)
+        relf = keep.tile([P, 2, 4], BF16, name="relf", align_bytes=64)
         w_bytes = keep.tile([P, 2 * R * F], U8, name="w_bytes", align_bytes=64)
         w_scale = keep.tile([P, R * F], F32, name="w_scale", align_bytes=64)
         w_val = keep.tile([P, 2 * R * F], BF16, name="w_val", align_bytes=64)
@@ -72,10 +85,12 @@ def tile_relationalgraphconvolution_pa_kernel(
         codes = {}
         scales = {}
         mx = {}
-        rs = {}
+        rep = {}
+        sbank = {}
+        sums = {}
         supn = {}
-        supr = {}
-        sgrp = {}
+        sgn = {}
+        sgr = {}
         scodes = {}
         sscales = {}
         obank = {}
@@ -91,40 +106,41 @@ def tile_relationalgraphconvolution_pa_kernel(
                     in_=adj[0, r0 : r0 + n, it * P : (it + 1) * P, :].rearrange("r i j -> i r j"),
                 )
 
-        def load_weight_bytes(h, f0, width):
-            c0 = h * R * F + f0 * R
-            rows = Wb_bytes[h * P : (h + 1) * P, :].rearrange("n (r f) -> n r f", f=F)
+        def load_features():
+            runs = node_features[0].rearrange("(c b u x e) d -> c u b x (e d)", c=2, u=2, x=8, e=2)
+            for c in range(2):
+                for u in range(2):
+                    nc.sync.dma_start(out=nf_raw[:, c, u * 2 * DE : (u + 1) * 2 * DE], in_=runs[c, u])
             nc.sync.dma_start(
-                out=w_bytes[:, c0 : c0 + R * width].rearrange("p (r d) -> p r d", d=width),
-                in_=rows[:, :, f0 : f0 + width],
+                out=nf_raw[:, 2:4, :], in_=node_features[0].rearrange("(c p t) d -> p c (t d)", p=P, t=4)
             )
 
-        def load_weight_scale(f0, width):
+        def load_weights(pair):
+            r0, n, f0, width = (0, R, DE, DR) if pair == 2 else (pair * 8, 8, 0, DE)
+            for h in range(2):
+                c0 = h * R * F + pair * 1024
+                rows = Wb_bytes[h * P : (h + 1) * P, :].rearrange("n (r f) -> n r f", f=F)
+                nc.sync.dma_start(
+                    out=w_bytes[:, c0 : c0 + 1024].rearrange("p (r d) -> p r d", d=width),
+                    in_=rows[:, r0 : r0 + n, f0 : f0 + width],
+                )
             sc = Wb_scale.rearrange("o (r f) -> (o r) f", f=F)
             nc.sync.dma_start(
-                out=w_scale[:, f0 * R : f0 * R + R * width].rearrange("p (r d) -> p r d", d=width),
-                in_=sc[:, f0 : f0 + width].partition_broadcast(P),
+                out=w_scale[:, pair * 1024 : (pair + 1) * 1024].rearrange("p (r d) -> p r d", d=width),
+                in_=sc[r0 : r0 + n, f0 : f0 + width].partition_broadcast(P),
             )
 
-        def open_step(s):
-            it, g = s // GROUPS, s % GROUPS
-            if g == 0:
-                rs[it] = late.tile([P, R], F32, name="rs")
-                supn[it] = three.tile([P, R * DE], BF16, name="supn", align_bytes=64)
-                supr[it] = three.tile([P, R * DR], BF16, name="supr", align_bytes=64)
-            perm[s] = three.tile([P, RG * N], BF16, name="perm", align_bytes=64)
-
-        def reorder(s, a):
-            it, g = s // GROUPS, s % GROUPS
-            r = g * RG + a
-            dst = perm[s][:, a * N : (a + 1) * N].rearrange("p (u q f) -> p u q f", u=2, f=16)
+        def row_sum(s, a):
+            col = s * RG + a
+            perm[col] = permp.tile([P, N], BF16, name="perm", align_bytes=64)
+            dst = perm[col][:].rearrange("p (u q f) -> p u q f", u=2, f=16)
             src = raw[s][:, a, :].rearrange("p (q u f) -> p u q f", u=2, f=16)
-            if a == RG - 1 and s in SCALAR_SUMS:
+            if on_scalar(s, a):
                 nc.scalar.activation(
                     out=dst,
                     in_=src,
                     func=mybir.ActivationFunctionType.Copy,
-                    accum_out=rs[it][:, r : r + 1],
+                    accum_out=rs[:, col : col + 1],
                 )
             else:
                 nc.vector.tensor_scalar(
@@ -134,33 +150,26 @@ def tile_relationalgraphconvolution_pa_kernel(
                     scalar2=None,
                     op0=MULT,
                     op1=ADD,
-                    accum_out=rs[it][:, r : r + 1],
+                    accum_out=rs[:, col : col + 1],
                 )
 
-        def relation_part(s, a, n):
-            it, g = s // GROUPS, s % GROUPS
-            r0 = g * RG + a
-            cols = slice(r0 * DR, (r0 + n) * DR)
-            nc.gpsimd.tensor_tensor(
-                out=supr[it][:, cols].rearrange("p (r d) -> p r d", d=DR),
-                in0=relf[:, cols].rearrange("p (r d) -> p r d", d=DR),
-                in1=rs[it][:, r0 : r0 + n].unsqueeze(2).to_broadcast([P, n, DR]),
-                op=MULT,
+        def turn(s, a, copy=nc.scalar.copy):
+            if a == 0:
+                grp[s] = three.tile([P, RG * N], BF16, name="grp", align_bytes=64)
+            bank = xtp.tile([P, 512], F32, name="xt")
+            for c in range(2):
+                for u in range(2):
+                    k0 = (c * 2 + u) * P
+                    if on_tensor(s, a):
+                        src = raw[s][:, a, :].bitcast(F32)[:, c * 256 + u : (c + 1) * 256 : 2]
+                    else:
+                        w0 = u * 256 + c * P
+                        src = perm[s * RG + a][:].bitcast(F32)[:, w0 : w0 + P]
+                    nc.tensor.transpose(bank[:, k0 : k0 + P], src, ident[:])
+            copy(
+                out=grp[s][:, a * N : (a + 1) * N].bitcast(F32).rearrange("p (c i u) -> p c i u", c=2, u=2),
+                in_=bank[:].rearrange("p (c u i) -> p c i u", c=2, u=2),
             )
-
-        def turn(s):
-            grp[s] = three.tile([P, RG * N], BF16, name="grp", align_bytes=64)
-            for a in range(RG):
-                bank = xtp.tile([P, 512], F32, name="xt")
-                for c in range(2):
-                    for u in range(2):
-                        k0 = (c * 2 + u) * P
-                        w0 = a * 512 + u * 256 + c * P
-                        nc.tensor.transpose(bank[:, k0 : k0 + P], perm[s][:].bitcast(F32)[:, w0 : w0 + P], ident[:])
-                nc.scalar.copy(
-                    out=grp[s][:, a * N : (a + 1) * N].bitcast(F32).rearrange("p (c i u) -> p c i u", c=2, u=2),
-                    in_=bank[:].rearrange("p (c u i) -> p c i u", c=2, u=2),
-                )
 
         def quantise(s, a0=0, n=RG):
             if a0 == 0:
@@ -173,86 +182,141 @@ def tile_relationalgraphconvolution_pa_kernel(
                 in_=grp[s][:, a0 * N : (a0 + n) * N],
             )
 
-        def aggregate(s, a0=0, n=RG):
+        def aggregate(s, a0, n):
             if a0 == 0:
                 mx[s] = mxp.tile([P, RG * DE], F32, name="mx")
             for a in range(a0, a0 + n):
                 for c in range(2):
                     cols = slice(a * 256 + c * P, a * 256 + (c + 1) * P)
-                    nf_cols = slice(c * DE, (c + 1) * DE)
+                    f0 = (c + 2) * DE if on_tensor(s, a) else c * DE
                     nc.tensor.matmul_mx(
                         out=mx[s][:, a * DE : (a + 1) * DE],
                         lhsT=codes[s][:, cols].bitcast(FP8X4),
                         lhsT_scale=scales[s][:, cols],
-                        rhs=nf_codes[:, nf_cols].bitcast(FP8X4),
-                        rhs_scale=nf_scales[:, nf_cols],
+                        rhs=nf_codes[:, f0 : f0 + DE].bitcast(FP8X4),
+                        rhs_scale=nf_scales[:, f0 : f0 + DE],
                         start=(c == 0),
                         stop=(c == 1),
                     )
 
-        def keep_supports(s, a0=0, n=RG):
-            it, g = s // GROUPS, s % GROUPS
-            dst = supn[it][:, g * 512 : (g + 1) * 512].rearrange("p (u q e) -> p u q e", u=2, e=2)
-            nc.scalar.copy(
+        def keep_supports(s, a0=0, n=RG, copy=nc.scalar.copy):
+            hh, g = s // 2, s % 2
+            if g == 0 and a0 == 0:
+                supn[hh] = three.tile([P, 1024], BF16, name="supn", align_bytes=64)
+            dst = supn[hh][:, g * 512 : (g + 1) * 512].rearrange("p (u q e) -> p u q e", u=2, e=2)
+            copy(
                 out=dst[:, :, a0 * 32 : (a0 + n) * 32, :],
                 in_=mx[s][:, a0 * DE : (a0 + n) * DE].rearrange("p (q u e) -> p u q e", u=2, e=2),
             )
 
-        def turn_supports(it, q0, n, copy=nc.scalar.copy):
-            if q0 == 0:
-                sgrp[it] = work.tile([P, 6 * 512], BF16, name="sgrp", align_bytes=64)
+        def turn_supports(hh, g0=0, n=2, copy=nc.scalar.copy):
+            if g0 == 0:
+                sgn[hh] = work.tile([P, 1024], BF16, name="sgn", align_bytes=64)
             bank = xtp.tile([P, 512], F32, name="xt")
             for b in range(n):
                 for u in range(2):
                     k0 = (b * 2 + u) * P
-                    q = q0 + b
-                    if q < 4:
-                        w0 = q * 256 + u * P
-                        src = supn[it][:].bitcast(F32)[:, w0 : w0 + P]
-                    else:
-                        w0 = (q - 4) * 256
-                        src = supr[it][:].bitcast(F32)[:, w0 + u : w0 + 256 : 2]
-                    nc.tensor.transpose(bank[:, k0 : k0 + P], src, ident[:])
+                    w0 = (g0 + b) * 256 + u * P
+                    nc.tensor.transpose(bank[:, k0 : k0 + P], supn[hh][:].bitcast(F32)[:, w0 : w0 + P], ident[:])
             copy(
-                out=sgrp[it][:, q0 * 512 : (q0 + n) * 512]
+                out=sgn[hh][:, g0 * 512 : (g0 + n) * 512]
                 .bitcast(F32)
                 .rearrange("p (b i u) -> p b i u", b=n, u=2),
                 in_=bank[:, 0 : n * 256].rearrange("p (b u i) -> p b i u", b=n, u=2),
             )
 
-        def quantise_supports(it, q0, n):
-            if q0 == 0:
-                scodes[it] = late.tile([P, 6 * P], U32, name="scodes", align_bytes=64)
-                sscales[it] = late.tile([P, 6 * P], U8, name="sscales", align_bytes=64)
-            cols = slice(q0 * P, (q0 + n) * P)
-            nc.vector.quantize_mx(
-                out=scodes[it][:, cols].bitcast(FP8X4),
-                scales=sscales[it][:, cols],
-                in_=sgrp[it][:, q0 * 512 : (q0 + n) * 512],
+        def spread_sums(hh):
+            rep[hh] = work.tile([P, P], F32, name="rep", align_bytes=64)
+            nc.gpsimd.tensor_scalar(
+                out=rep[hh][:].rearrange("p (r q) -> p r q", q=16),
+                in0=rs[:, hh * 8 : (hh + 1) * 8].unsqueeze(2).to_broadcast([P, 8, 16]),
+                scalar1=1.0,
+                scalar2=0.0,
+                op0=MULT,
+                op1=ADD,
             )
 
-        def project(it, passes, first, last):
-            if first:
-                obank[it] = outp.tile([P, NB], F32, name="o")
-            for j, q in enumerate(passes):
-                cols = slice(q * P, (q + 1) * P)
-                w_cols = slice(q * NB, (q + 1) * NB)
-                nc.tensor.matmul_mx(
-                    out=obank[it][:],
-                    lhsT=scodes[it][:, cols].bitcast(FP8X4),
-                    lhsT_scale=sscales[it][:, cols],
-                    rhs=w_codes[:, w_cols].bitcast(FP8X4),
-                    rhs_scale=w_scales[:, w_cols],
-                    start=(first and j == 0),
-                    stop=(last and j == len(passes) - 1),
+        def tensor_sum(hh, c):
+            if c == 0:
+                sbank[hh] = sump.tile([P, 256], F32, name="sb")
+            c0 = TENSOR_A * N + c * 512
+            words = grp[2 * hh + 1][:, c0 : c0 + 512].rearrange("p (i u e) -> p u i e", u=2, e=2)
+            for u in range(2):
+                nc.tensor.matmul(
+                    sbank[hh][:].rearrange("p (i e) -> p i e", e=2),
+                    lhsT=mask[:],
+                    rhs=words[:, u],
+                    start=(c == 0 and u == 0),
+                    stop=False,
                 )
+
+        def turn_sums(hh):
+            if on_tensor(2 * hh + 1, TENSOR_A):
+                nc.tensor.matmul(sbank[hh][:, 0:256:2], lhsT=rep[hh][:], rhs=ident[:], start=False, stop=True)
+            else:
+                sbank[hh] = sump.tile([P, 256], F32, name="sb")
+                nc.tensor.matmul(sbank[hh][:, 0:P], lhsT=rep[hh][:], rhs=ident[:], start=True, stop=True)
+
+        def relation_part(hh):
+            sgr[hh] = work.tile([P, 512], BF16, name="sgr", align_bytes=64)
+            if on_tensor(2 * hh + 1, TENSOR_A):
+                sums[hh] = work.tile([P, P], F32, name="sums", align_bytes=64)
+                nc.vector.tensor_reduce(
+                    out=sums[hh][:],
+                    in_=sbank[hh][:].rearrange("p (i e) -> p i e", e=2),
+                    axis=mybir.AxisListType.X,
+                    op=ADD,
+                )
+                engine, src = nc.gpsimd, sums[hh][:]
+            else:
+                engine, src = nc.vector, sbank[hh][:, 0:P]
+            engine.tensor_tensor(
+                out=sgr[hh][:].rearrange("p (i t) -> p i t", t=4),
+                in0=src.unsqueeze(2).to_broadcast([P, P, 4]),
+                in1=relf[:, hh % 2, :].unsqueeze(1).to_broadcast([P, P, 4]),
+                op=MULT,
+            )
+
+        def quantise_relation(hh):
+            scodes[hh] = late.tile([P, 3 * P], U32, name="scodes", align_bytes=64)
+            sscales[hh] = late.tile([P, 3 * P], U8, name="sscales", align_bytes=64)
+            nc.vector.quantize_mx(
+                out=scodes[hh][:, 2 * P : 3 * P].bitcast(FP8X4), scales=sscales[hh][:, 2 * P : 3 * P], in_=sgr[hh][:]
+            )
+
+        def quantise_nodes(hh, g0=0, n=2):
+            cols = slice(g0 * P, (g0 + n) * P)
+            nc.vector.quantize_mx(
+                out=scodes[hh][:, cols].bitcast(FP8X4),
+                scales=sscales[hh][:, cols],
+                in_=sgn[hh][:, g0 * 512 : (g0 + n) * 512],
+            )
+
+        def project(hh, j):
+            it, h = hh // 2, hh % 2
+            first = h == 0 and j == 2
+            if first:
+                if it == IT - 1:
+                    obank[it] = xtp.tile([P, 512], F32, name="xt")
+                else:
+                    obank[it] = outp.tile([P, NB], F32, name="o")
+            q = 4 + h if j == 2 else 2 * h + j
+            nc.tensor.matmul_mx(
+                out=obank[it][:, 0:NB],
+                lhsT=scodes[hh][:, j * P : (j + 1) * P].bitcast(FP8X4),
+                lhsT_scale=sscales[hh][:, j * P : (j + 1) * P],
+                rhs=w_codes[:, q * NB : (q + 1) * NB].bitcast(FP8X4),
+                rhs_scale=w_scales[:, q * NB : (q + 1) * NB],
+                start=first,
+                stop=(h == 1 and j == 1),
+            )
 
         def store(it):
             res = work.tile([P, NB], F32, name="res", align_bytes=64)
-            nc.scalar.copy(out=res[:], in_=obank[it][:])
+            nc.scalar.copy(out=res[:], in_=obank[it][:, 0:NB])
             nc.sync.dma_start(out=out[0, it * P : (it + 1) * P, :], in_=res[:])
 
-        def weight_values(h, pair):
+        def weight_values(pair, h):
             c0 = h * R * F + pair * 1024
             nc.vector.tensor_tensor(
                 out=w_val[:, c0 : c0 + 1024],
@@ -283,105 +347,98 @@ def tile_relationalgraphconvolution_pa_kernel(
             )
 
         load(0, 4)
-        nc.sync.dma_start(
-            out=nf_raw[:], in_=node_features[0].rearrange("(c p t) d -> p c t d", p=P, t=4)
-        )
+        load_features()
         load(1, 2)
-        nc.sync.dma_start(
-            out=relf[:], in_=relation_features[0].rearrange("r d -> (r d)").partition_broadcast(P)
-        )
-        for s in range(2, PREFETCH):
+        load(2, 2)
+        nc.sync.dma_start(out=relf[:], in_=relation_features[0].rearrange("(h r) (q t) -> (r q) h t", h=2, t=4))
+        for s in range(3, PREFETCH):
             load(s)
 
-        open_step(0)
-        for a in range(RG):
-            reorder(0, a)
-        relation_part(0, 0, RG)
-        for c in range(2):
-            bank = xtp.tile([P, 512], F32, name="xt")
-            for u in range(2):
-                for h in range(2):
-                    nc.tensor.matmul(
-                        bank[:, u * 256 : (u + 1) * 256],
-                        lhsT=select[:, 2 * u + h, :],
-                        rhs=nf_raw[:, c, 2 * h : 2 * h + 2, :].rearrange("p e d -> p (e d)"),
-                        start=(h == 0),
-                        stop=(h == 1),
-                    )
-            nc.scalar.copy(out=nf_grp[:, c], in_=bank[:].rearrange("p (t d) -> p d t", t=4))
-        nc.vector.quantize_mx(
-            out=nf_codes[:].bitcast(FP8X4),
-            scales=nf_scales[:],
-            in_=nf_grp[:].rearrange("p c d t -> p (c d t)"),
-        )
+        for col in range(2 * RG - 1):
+            if not on_tensor(col // RG, col % RG):
+                row_sum(col // RG, col % RG)
 
-        project_at = {}
-        for it in range(IT - 1):
-            project_at[max(4 * it + 8, 21 + it)] = it
-        weight_loads = {
-            2: (load_weight_bytes, (0, 0, DE)),
-            3: (load_weight_bytes, (0, DE, DR)),
-            4: (load_weight_bytes, (1, 0, DE)),
-            5: (load_weight_bytes, (1, DE, DR)),
-            6: (load_weight_scale, (0, DE)),
-            8: (load_weight_scale, (DE, DR)),
-        }
+        pair_order = (2, 0, 1)
+        project_at = {max(2 * hh + 7, hh + FIRST_PROJECT): hh for hh in range(HALVES)}
 
         for s in range(STEPS):
             if s + PREFETCH < STEPS:
                 load(s + PREFETCH)
-            if s in weight_loads:
-                fn, args = weight_loads[s]
-                fn(*args)
-            if s + 1 < STEPS:
-                open_step(s + 1)
-                reorder(s + 1, 0)
-            if s >= 1:
-                quantise(s - 1)
-            turn(s)
-            for q0, at in ((0, 4), (4, 5), (2, 6)):
-                if s >= at and (s - at) % 4 == 0:
-                    turn_supports((s - at) // 4, q0, 2)
-            if 16 <= s < 19:
-                turn_weights(2 * (s - 16))
-                turn_weights(2 * (s - 16) + 1)
+            if s < 3:
+                load_weights(pair_order[s])
             if s >= 2:
-                aggregate(s - 2)
+                quantise(s - 1)
+            if s >= 4 and s % 2 == 0:
+                quantise_relation((s - 4) // 2)
+            if s >= 5 and s % 2 == 1:
+                quantise_nodes((s - 5) // 2)
+            if W0 + 4 <= s < W0 + 10 and (s - W0) % 2 == 0:
+                quantise_weights(pair_order[(s - W0 - 4) // 2])
+            if W0 <= s < W0 + 6:
+                weight_values(pair_order[(s - W0) // 2], (s - W0) % 2)
+            for half in range(2):
+                turn(s, 2 * half)
+                turn(s, 2 * half + 1, nc.vector.tensor_copy if 2 * s + half >= VECTOR_EXITS else nc.scalar.copy)
+                if half == 0 and W0 + 2 <= s < W0 + 8:
+                    turn_weights(2 * pair_order[(s - W0 - 2) // 2] + (s - W0) % 2)
+                if half == 1 and s >= 4 and s % 2 == 0:
+                    turn_supports((s - 4) // 2)
+                if s >= 2 and s % 2 == 0 and on_tensor(s - 1, TENSOR_A):
+                    tensor_sum((s - 2) // 2, half)
+                if half == 0 and s >= 3 and s % 2 == 1:
+                    turn_sums((s - 3) // 2)
+                if s >= 2:
+                    aggregate(s - 2, 2 * half, 2)
+                if s in project_at:
+                    for j in ((2,), (0, 1))[half]:
+                        project(project_at[s], j)
+            if s == 0:
+                for v in range(2):
+                    nc.scalar.copy(
+                        out=nf_grp[:, v * 1024 : (v + 1) * 1024].rearrange("p (c d t) -> p c d t", c=2, t=4),
+                        in_=nf_raw[:, 2 * v : 2 * v + 2, :].rearrange("p c (t d) -> p c d t", t=4),
+                    )
+            if s >= 2:
                 keep_supports(s - 2)
-            if 10 <= s < 16:
-                weight_values((s - 10) % 2, (s - 10) // 2)
-            if 17 <= s < 20:
-                quantise_weights(s - 17)
-            for q0, at in ((0, 5), (4, 6), (2, 7)):
-                if s >= at and (s - at) % 4 == 0:
-                    quantise_supports((s - at) // 4, q0, 2)
+            if s in project_at and project_at[s] % 2 == 1:
+                store(project_at[s] // 2)
+            if s >= 3 and s % 2 == 1:
+                relation_part((s - 3) // 2)
             if s + 1 < STEPS:
-                reorder(s + 1, 1)
-                relation_part(s + 1, 0, 2)
-                reorder(s + 1, 2)
-                reorder(s + 1, 3)
-                relation_part(s + 1, 2, 2)
-            if s in project_at:
-                project(project_at[s], range(6), True, True)
-                store(project_at[s])
+                row_sum(s + 1, RG - 1)
+                if s % 2 == 0:
+                    spread_sums(s // 2)
+            if s == 0:
+                quantise(0)
+                nc.vector.quantize_mx(out=nf_codes[:].bitcast(FP8X4), scales=nf_scales[:], in_=nf_grp[:])
+            if s + 2 < STEPS:
+                for a in range(RG - 1):
+                    if not on_tensor(s + 2, a):
+                        row_sum(s + 2, a)
 
-        it, s = IT - 1, STEPS - 1
-        project(it - 1, range(6), True, True)
-        store(it - 1)
-        aggregate(s - 1)
+        s, hh = STEPS - 1, HALVES - 1
+        aggregate(s - 1, 0, RG)
+        turn_sums(hh)
+        for j in (2, 0, 1):
+            project(hh - 2, j)
+        quantise(s, 0, 2)
+        quantise(s, 2, 2)
         keep_supports(s - 1)
-        for a in range(RG):
-            quantise(s, a, 1)
-        turn_supports(it, 0, 2, nc.vector.tensor_copy)
-        turn_supports(it, 4, 2, nc.vector.tensor_copy)
-        aggregate(s)
+        turn_supports(hh - 1)
+        aggregate(s, 0, RG)
+        quantise_relation(hh - 1)
+        relation_part(hh)
+        turn_supports(hh, 0, 1, nc.vector.tensor_copy)
         keep_supports(s)
-        turn_supports(it, 2, 1, nc.vector.tensor_copy)
-        quantise_supports(it, 0, 2)
-        quantise_supports(it, 4, 2)
-        quantise_supports(it, 2, 1)
-        project(it, (0, 1, 4, 5, 2), True, False)
-        turn_supports(it, 3, 1)
-        quantise_supports(it, 3, 1)
-        project(it, (3,), False, True)
-        store(it)
+        quantise_nodes(hh - 1)
+        quantise_relation(hh)
+        turn_supports(hh, 1, 1)
+        quantise_nodes(hh, 0, 1)
+        store(IT - 2)
+        for j in (2, 0, 1):
+            project(hh - 1, j)
+        project(hh, 2)
+        project(hh, 0)
+        quantise_nodes(hh, 1, 1)
+        project(hh, 1)
+        store(IT - 1)

@@ -16,11 +16,12 @@ GROUPS = R // RG
 STEPS = IT * GROUPS
 HALVES = STEPS // 2
 PREFETCH = 5
-TENSOR_A = 1
+TENSOR_A = 0
+SCALAR_A = 1
 W0 = 4
-VECTOR_EXITS = 61
+VECTOR_EXITS = 63
 FIRST_PROJECT = 12
-SCALAR_STEPS = tuple(range(4, 12)) + tuple(range(12, 26, 2))
+SCALAR_STEPS = tuple(range(4, 11)) + tuple(range(12, 32, 2))
 
 F32 = mybir.dt.float32
 BF16 = mybir.dt.bfloat16
@@ -35,11 +36,11 @@ FLOPS = 2 * (R * N * N * DE + N * R * F * NB)
 
 
 def on_tensor(s, a):
-    return a == TENSOR_A and s % 2 == 1 and s < STEPS - 1
+    return a == TENSOR_A and s % 2 == 0 and s < STEPS - 2
 
 
 def on_scalar(s, a):
-    return a == 0 and s in SCALAR_STEPS
+    return (a == SCALAR_A and s in SCALAR_STEPS) or (s, a) == (1, 2)
 
 
 def tile_relationalgraphconvolution_pa_kernel(
@@ -52,7 +53,8 @@ def tile_relationalgraphconvolution_pa_kernel(
         permp = ctx.enter_context(tc.tile_pool(name="permp", bufs=12))
         work = ctx.enter_context(tc.tile_pool(name="work", bufs=2))
         three = ctx.enter_context(tc.tile_pool(name="three", bufs=3))
-        late = ctx.enter_context(tc.tile_pool(name="late", bufs=6))
+        four = ctx.enter_context(tc.tile_pool(name="four", bufs=4))
+        late = ctx.enter_context(tc.tile_pool(name="late", bufs=7))
         xtp = ctx.enter_context(tc.psum_pool(name="xtp", bufs=4))
         mxp = ctx.enter_context(tc.psum_pool(name="mxp", bufs=2))
         outp = ctx.enter_context(tc.psum_pool(name="outp", bufs=1))
@@ -64,7 +66,7 @@ def tile_relationalgraphconvolution_pa_kernel(
         rs = keep.tile([P, IT * R], F32, name="rs", align_bytes=64)
         nc.vector.memset(rs[:], 0.0)
         mask = keep.tile([P, P], BF16, name="mask", align_bytes=64)
-        m0 = (RG + TENSOR_A) * 16
+        m0 = TENSOR_A * 16
         nc.vector.memset(mask[:], 0.0)
         nc.vector.memset(mask[:, m0 : m0 + 16], 1.0)
         nf_raw = keep.tile([P, 4, 4 * DE], BF16, name="nf_raw", align_bytes=64)
@@ -153,9 +155,9 @@ def tile_relationalgraphconvolution_pa_kernel(
                     accum_out=rs[:, col : col + 1],
                 )
 
-        def turn(s, a, copy=nc.scalar.copy):
+        def turn(s, a):
             if a == 0:
-                grp[s] = three.tile([P, RG * N], BF16, name="grp", align_bytes=64)
+                grp[s] = four.tile([P, RG * N], BF16, name="grp", align_bytes=64)
             bank = xtp.tile([P, 512], F32, name="xt")
             for c in range(2):
                 for u in range(2):
@@ -166,6 +168,9 @@ def tile_relationalgraphconvolution_pa_kernel(
                         w0 = u * 256 + c * P
                         src = perm[s * RG + a][:].bitcast(F32)[:, w0 : w0 + P]
                     nc.tensor.transpose(bank[:, k0 : k0 + P], src, ident[:])
+            return bank
+
+        def empty(s, a, bank, copy=nc.scalar.copy):
             copy(
                 out=grp[s][:, a * N : (a + 1) * N].bitcast(F32).rearrange("p (c i u) -> p c i u", c=2, u=2),
                 in_=bank[:].rearrange("p (c u i) -> p c i u", c=2, u=2),
@@ -240,7 +245,7 @@ def tile_relationalgraphconvolution_pa_kernel(
             if c == 0:
                 sbank[hh] = sump.tile([P, 256], F32, name="sb")
             c0 = TENSOR_A * N + c * 512
-            words = grp[2 * hh + 1][:, c0 : c0 + 512].rearrange("p (i u e) -> p u i e", u=2, e=2)
+            words = grp[2 * hh][:, c0 : c0 + 512].rearrange("p (i u e) -> p u i e", u=2, e=2)
             for u in range(2):
                 nc.tensor.matmul(
                     sbank[hh][:].rearrange("p (i e) -> p i e", e=2),
@@ -251,29 +256,28 @@ def tile_relationalgraphconvolution_pa_kernel(
                 )
 
         def turn_sums(hh):
-            if on_tensor(2 * hh + 1, TENSOR_A):
+            if on_tensor(2 * hh, TENSOR_A):
                 nc.tensor.matmul(sbank[hh][:, 0:256:2], lhsT=rep[hh][:], rhs=ident[:], start=False, stop=True)
             else:
                 sbank[hh] = sump.tile([P, 256], F32, name="sb")
                 nc.tensor.matmul(sbank[hh][:, 0:P], lhsT=rep[hh][:], rhs=ident[:], start=True, stop=True)
 
-        def relation_part(hh):
-            sgr[hh] = work.tile([P, 512], BF16, name="sgr", align_bytes=64)
-            if on_tensor(2 * hh + 1, TENSOR_A):
-                sums[hh] = work.tile([P, P], F32, name="sums", align_bytes=64)
-                nc.vector.tensor_reduce(
-                    out=sums[hh][:],
-                    in_=sbank[hh][:].rearrange("p (i e) -> p i e", e=2),
-                    axis=mybir.AxisListType.X,
-                    op=ADD,
-                )
-                engine, src = nc.gpsimd, sums[hh][:]
-            else:
-                engine, src = nc.vector, sbank[hh][:, 0:P]
+        def collect_sums(hh):
+            sums[hh] = work.tile([P, P], F32, name="sums", align_bytes=64)
+            nc.vector.tensor_reduce(
+                out=sums[hh][:],
+                in_=sbank[hh][:].rearrange("p (i e) -> p i e", e=2),
+                axis=mybir.AxisListType.X,
+                op=ADD,
+            )
+
+        def relation_part(hh, src, engine, i0=0, n=P):
+            if i0 == 0:
+                sgr[hh] = work.tile([P, 512], BF16, name="sgr", align_bytes=64)
             engine.tensor_tensor(
-                out=sgr[hh][:].rearrange("p (i t) -> p i t", t=4),
-                in0=src.unsqueeze(2).to_broadcast([P, P, 4]),
-                in1=relf[:, hh % 2, :].unsqueeze(1).to_broadcast([P, P, 4]),
+                out=sgr[hh][:, i0 * 4 : (i0 + n) * 4].rearrange("p (i t) -> p i t", t=4),
+                in0=src[:, i0 : i0 + n].unsqueeze(2).to_broadcast([P, n, 4]),
+                in1=relf[:, hh % 2, :].unsqueeze(1).to_broadcast([P, n, 4]),
                 op=MULT,
             )
 
@@ -355,90 +359,106 @@ def tile_relationalgraphconvolution_pa_kernel(
             load(s)
 
         for col in range(2 * RG - 1):
-            if not on_tensor(col // RG, col % RG):
+            if not on_tensor(col // RG, col % RG) and not on_scalar(col // RG, col % RG):
                 row_sum(col // RG, col % RG)
 
+        nc.gpsimd.tensor_scalar(
+            out=nf_grp[:].rearrange("p (c d t) -> p c d t", c=4, t=4),
+            in0=nf_raw[:].rearrange("p c (t d) -> p c d t", t=4),
+            scalar1=1.0,
+            scalar2=0.0,
+            op0=MULT,
+            op1=ADD,
+        )
+
         pair_order = (2, 0, 1)
-        project_at = {max(2 * hh + 7, hh + FIRST_PROJECT): hh for hh in range(HALVES)}
+        project_at = {max(2 * hh + 7, 3 * hh // 2 + FIRST_PROJECT): hh for hh in range(HALVES)}
 
         for s in range(STEPS):
             if s + PREFETCH < STEPS:
                 load(s + PREFETCH)
             if s < 3:
                 load_weights(pair_order[s])
+            if s == 1:
+                nc.vector.quantize_mx(out=nf_codes[:].bitcast(FP8X4), scales=nf_scales[:], in_=nf_grp[:])
             if s >= 2:
                 quantise(s - 1)
             if s >= 4 and s % 2 == 0:
                 quantise_relation((s - 4) // 2)
-            if s >= 5 and s % 2 == 1:
-                quantise_nodes((s - 5) // 2)
+            if s >= 6 and s % 2 == 0:
+                quantise_nodes((s - 6) // 2)
             if W0 + 4 <= s < W0 + 10 and (s - W0) % 2 == 0:
                 quantise_weights(pair_order[(s - W0 - 4) // 2])
             if W0 <= s < W0 + 6:
                 weight_values(pair_order[(s - W0) // 2], (s - W0) % 2)
             for half in range(2):
-                turn(s, 2 * half)
-                turn(s, 2 * half + 1, nc.vector.tensor_copy if 2 * s + half >= VECTOR_EXITS else nc.scalar.copy)
+                a = 2 * half
+                banks = [turn(s, a), turn(s, a + 1)]
+                for b in range(2):
+                    to_vector = b == 1 and 2 * s + half >= VECTOR_EXITS
+                    empty(s, a + b, banks[b], nc.vector.tensor_copy if to_vector else nc.scalar.copy)
                 if half == 0 and W0 + 2 <= s < W0 + 8:
                     turn_weights(2 * pair_order[(s - W0 - 2) // 2] + (s - W0) % 2)
-                if half == 1 and s >= 4 and s % 2 == 0:
-                    turn_supports((s - 4) // 2)
-                if s >= 2 and s % 2 == 0 and on_tensor(s - 1, TENSOR_A):
+                if half == 1 and s >= 5 and s % 2 == 1:
+                    turn_supports((s - 5) // 2)
+                if half == 0 and s >= 3:
+                    keep_supports(s - 3)
+                store_half = 0 if s in project_at else 1
+                if half == store_half and s - 1 in project_at and project_at[s - 1] % 2 == 1:
+                    store(project_at[s - 1] // 2)
+                if half == 1 and s == 0:
+                    row_sum(1, 2)
+                if half == 1 and s + 2 < STEPS and on_scalar(s + 2, SCALAR_A):
+                    row_sum(s + 2, SCALAR_A)
+                if s >= 2 and s % 2 == 0 and on_tensor(s - 2, TENSOR_A):
                     tensor_sum((s - 2) // 2, half)
                 if half == 0 and s >= 3 and s % 2 == 1:
                     turn_sums((s - 3) // 2)
                 if s >= 2:
-                    aggregate(s - 2, 2 * half, 2)
+                    aggregate(s - 2, a, 2)
                 if s in project_at:
                     for j in ((2,), (0, 1))[half]:
                         project(project_at[s], j)
-            if s == 0:
-                for v in range(2):
-                    nc.scalar.copy(
-                        out=nf_grp[:, v * 1024 : (v + 1) * 1024].rearrange("p (c d t) -> p c d t", c=2, t=4),
-                        in_=nf_raw[:, 2 * v : 2 * v + 2, :].rearrange("p c (t d) -> p c d t", t=4),
-                    )
-            if s >= 2:
-                keep_supports(s - 2)
-            if s in project_at and project_at[s] % 2 == 1:
-                store(project_at[s] // 2)
             if s >= 3 and s % 2 == 1:
-                relation_part((s - 3) // 2)
+                hh = (s - 3) // 2
+                collect_sums(hh)
+                if s + 1 < STEPS:
+                    relation_part(hh, sums[hh], nc.gpsimd)
             if s + 1 < STEPS:
+                if s % 2 == 1:
+                    row_sum(s + 1, RG - 2)
                 row_sum(s + 1, RG - 1)
                 if s % 2 == 0:
                     spread_sums(s // 2)
             if s == 0:
                 quantise(0)
-                nc.vector.quantize_mx(out=nf_codes[:].bitcast(FP8X4), scales=nf_scales[:], in_=nf_grp[:])
             if s + 2 < STEPS:
-                for a in range(RG - 1):
-                    if not on_tensor(s + 2, a):
+                for a in range(RG - 2 + s % 2):
+                    if not on_tensor(s + 2, a) and not on_scalar(s + 2, a):
                         row_sum(s + 2, a)
 
         s, hh = STEPS - 1, HALVES - 1
-        aggregate(s - 1, 0, RG)
         turn_sums(hh)
+        aggregate(s - 1, 0, RG)
+        quantise(s, 0, 2)
+        relation_part(hh - 1, sums[hh - 1], nc.vector)
+        quantise(s, 2, 2)
+        keep_supports(s - 2)
+        keep_supports(s - 1)
+        aggregate(s, 0, RG)
+        turn_supports(hh - 1)
+        quantise_nodes(hh - 2)
+        relation_part(hh, sbank[hh], nc.vector)
+        keep_supports(s, copy=nc.vector.tensor_copy)
         for j in (2, 0, 1):
             project(hh - 2, j)
-        quantise(s, 0, 2)
-        quantise(s, 2, 2)
-        keep_supports(s - 1)
-        turn_supports(hh - 1)
-        aggregate(s, 0, RG)
+        turn_supports(hh)
         quantise_relation(hh - 1)
-        relation_part(hh)
-        turn_supports(hh, 0, 1, nc.vector.tensor_copy)
-        keep_supports(s)
         quantise_nodes(hh - 1)
         quantise_relation(hh)
-        turn_supports(hh, 1, 1)
-        quantise_nodes(hh, 0, 1)
         store(IT - 2)
-        for j in (2, 0, 1):
-            project(hh - 1, j)
-        project(hh, 2)
-        project(hh, 0)
-        quantise_nodes(hh, 1, 1)
-        project(hh, 1)
+        quantise_nodes(hh)
+        for half in range(2):
+            for j in (2, 0, 1):
+                project(hh - 1 + half, j)
         store(IT - 1)

@@ -20,7 +20,9 @@ TENSOR_A = 0
 SCALAR_A = 1
 W0 = 4
 VECTOR_EXITS = 63
-FIRST_PROJECT = 12
+FIRST_PROJECT = 13
+PROJECT_LAG = 9
+TURN_LAG = 5
 SCALAR_STEPS = tuple(range(4, 11)) + tuple(range(12, 32, 2))
 
 F32 = mybir.dt.float32
@@ -55,9 +57,7 @@ def tile_relationalgraphconvolution_pa_kernel(
         three = ctx.enter_context(tc.tile_pool(name="three", bufs=3))
         four = ctx.enter_context(tc.tile_pool(name="four", bufs=4))
         late = ctx.enter_context(tc.tile_pool(name="late", bufs=7))
-        xtp = ctx.enter_context(tc.psum_pool(name="xtp", bufs=4))
-        mxp = ctx.enter_context(tc.psum_pool(name="mxp", bufs=2))
-        outp = ctx.enter_context(tc.psum_pool(name="outp", bufs=1))
+        ring = ctx.enter_context(tc.psum_pool(name="ring", bufs=7))
         sump = ctx.enter_context(tc.psum_pool(name="sump", bufs=1))
         ctx.enter_context(tc.manual_schedule())
 
@@ -158,7 +158,7 @@ def tile_relationalgraphconvolution_pa_kernel(
         def turn(s, a):
             if a == 0:
                 grp[s] = four.tile([P, RG * N], BF16, name="grp", align_bytes=64)
-            bank = xtp.tile([P, 512], F32, name="xt")
+            bank = ring.tile([P, 512], F32, name="bank")
             for c in range(2):
                 for u in range(2):
                     k0 = (c * 2 + u) * P
@@ -189,7 +189,7 @@ def tile_relationalgraphconvolution_pa_kernel(
 
         def aggregate(s, a0, n):
             if a0 == 0:
-                mx[s] = mxp.tile([P, RG * DE], F32, name="mx")
+                mx[s] = ring.tile([P, 512], F32, name="bank")
             for a in range(a0, a0 + n):
                 for c in range(2):
                     cols = slice(a * 256 + c * P, a * 256 + (c + 1) * P)
@@ -217,7 +217,7 @@ def tile_relationalgraphconvolution_pa_kernel(
         def turn_supports(hh, g0=0, n=2, copy=nc.scalar.copy):
             if g0 == 0:
                 sgn[hh] = work.tile([P, 1024], BF16, name="sgn", align_bytes=64)
-            bank = xtp.tile([P, 512], F32, name="xt")
+            bank = ring.tile([P, 512], F32, name="bank")
             for b in range(n):
                 for u in range(2):
                     k0 = (b * 2 + u) * P
@@ -257,10 +257,12 @@ def tile_relationalgraphconvolution_pa_kernel(
 
         def turn_sums(hh):
             if on_tensor(2 * hh, TENSOR_A):
-                nc.tensor.matmul(sbank[hh][:, 0:256:2], lhsT=rep[hh][:], rhs=ident[:], start=False, stop=True)
+                nc.tensor.matmul(
+                    sbank[hh][:, 0:256:2], lhsT=rep[hh][:], rhs=ident[:], start=False, stop=True, is_transpose=True
+                )
             else:
                 sbank[hh] = sump.tile([P, 256], F32, name="sb")
-                nc.tensor.matmul(sbank[hh][:, 0:P], lhsT=rep[hh][:], rhs=ident[:], start=True, stop=True)
+                nc.tensor.transpose(sbank[hh][:, 0:P], rep[hh][:], ident[:])
 
         def collect_sums(hh):
             sums[hh] = work.tile([P, P], F32, name="sums", align_bytes=64)
@@ -300,10 +302,7 @@ def tile_relationalgraphconvolution_pa_kernel(
             it, h = hh // 2, hh % 2
             first = h == 0 and j == 2
             if first:
-                if it == IT - 1:
-                    obank[it] = xtp.tile([P, 512], F32, name="xt")
-                else:
-                    obank[it] = outp.tile([P, NB], F32, name="o")
+                obank[it] = ring.tile([P, 512], F32, name="bank")
             q = 4 + h if j == 2 else 2 * h + j
             nc.tensor.matmul_mx(
                 out=obank[it][:, 0:NB],
@@ -330,7 +329,7 @@ def tile_relationalgraphconvolution_pa_kernel(
             )
 
         def turn_weights(q):
-            bank = xtp.tile([P, 512], F32, name="xt")
+            bank = ring.tile([P, 512], F32, name="bank")
             words = w_val[:].bitcast(F32)
             for h in range(2):
                 for u in range(2):
@@ -372,7 +371,7 @@ def tile_relationalgraphconvolution_pa_kernel(
         )
 
         pair_order = (2, 0, 1)
-        project_at = {max(2 * hh + 7, 3 * hh // 2 + FIRST_PROJECT): hh for hh in range(HALVES)}
+        project_at = {max(4 * it + PROJECT_LAG, 2 * it + FIRST_PROJECT): it for it in range(IT)}
 
         for s in range(STEPS):
             if s + PREFETCH < STEPS:
@@ -385,40 +384,38 @@ def tile_relationalgraphconvolution_pa_kernel(
                 quantise(s - 1)
             if s >= 4 and s % 2 == 0:
                 quantise_relation((s - 4) // 2)
-            if s >= 6 and s % 2 == 0:
-                quantise_nodes((s - 6) // 2)
+            if s >= TURN_LAG + 1 and (s - TURN_LAG) % 2 == 1:
+                quantise_nodes((s - TURN_LAG - 1) // 2)
             if W0 + 4 <= s < W0 + 10 and (s - W0) % 2 == 0:
                 quantise_weights(pair_order[(s - W0 - 4) // 2])
             if W0 <= s < W0 + 6:
                 weight_values(pair_order[(s - W0) // 2], (s - W0) % 2)
-            for half in range(2):
-                a = 2 * half
-                banks = [turn(s, a), turn(s, a + 1)]
-                for b in range(2):
-                    to_vector = b == 1 and 2 * s + half >= VECTOR_EXITS
-                    empty(s, a + b, banks[b], nc.vector.tensor_copy if to_vector else nc.scalar.copy)
-                if half == 0 and W0 + 2 <= s < W0 + 8:
-                    turn_weights(2 * pair_order[(s - W0 - 2) // 2] + (s - W0) % 2)
-                if half == 1 and s >= 5 and s % 2 == 1:
-                    turn_supports((s - 5) // 2)
-                if half == 0 and s >= 3:
-                    keep_supports(s - 3)
-                store_half = 0 if s in project_at else 1
-                if half == store_half and s - 1 in project_at and project_at[s - 1] % 2 == 1:
-                    store(project_at[s - 1] // 2)
-                if half == 1 and s == 0:
-                    row_sum(1, 2)
-                if half == 1 and s + 2 < STEPS and on_scalar(s + 2, SCALAR_A):
+            if s >= 3 and s % 2 == 1:
+                turn_sums((s - 3) // 2)
+            for a in range(RG):
+                to_vector = a % 2 == 1 and 2 * s + a // 2 >= VECTOR_EXITS
+                empty(s, a, turn(s, a), nc.vector.tensor_copy if to_vector else nc.scalar.copy)
+                if a == 1 and s + 2 < STEPS and on_scalar(s + 2, SCALAR_A):
                     row_sum(s + 2, SCALAR_A)
-                if s >= 2 and s % 2 == 0 and on_tensor(s - 2, TENSOR_A):
-                    tensor_sum((s - 2) // 2, half)
-                if half == 0 and s >= 3 and s % 2 == 1:
-                    turn_sums((s - 3) // 2)
-                if s >= 2:
-                    aggregate(s - 2, a, 2)
-                if s in project_at:
-                    for j in ((2,), (0, 1))[half]:
-                        project(project_at[s], j)
+            if W0 + 2 <= s < W0 + 8:
+                turn_weights(2 * pair_order[(s - W0 - 2) // 2] + (s - W0) % 2)
+            if s >= TURN_LAG and (s - TURN_LAG) % 2 == 0:
+                turn_supports((s - TURN_LAG) // 2)
+            if s == 0:
+                row_sum(1, 2)
+            if s >= 2 and s % 2 == 0 and on_tensor(s - 2, TENSOR_A):
+                for c in range(2):
+                    tensor_sum((s - 2) // 2, c)
+            if s >= 2:
+                aggregate(s - 2, 0, RG)
+            if s in project_at:
+                for half in range(2):
+                    for j in (2, 0, 1):
+                        project(2 * project_at[s] + half, j)
+            if s >= 2:
+                keep_supports(s - 2)
+            if s in project_at:
+                store(project_at[s])
             if s >= 3 and s % 2 == 1:
                 hh = (s - 3) // 2
                 collect_sums(hh)
@@ -443,15 +440,15 @@ def tile_relationalgraphconvolution_pa_kernel(
         quantise(s, 0, 2)
         relation_part(hh - 1, sums[hh - 1], nc.vector)
         quantise(s, 2, 2)
-        keep_supports(s - 2)
         keep_supports(s - 1)
         aggregate(s, 0, RG)
         turn_supports(hh - 1)
         quantise_nodes(hh - 2)
         relation_part(hh, sbank[hh], nc.vector)
         keep_supports(s, copy=nc.vector.tensor_copy)
-        for j in (2, 0, 1):
-            project(hh - 2, j)
+        for half in range(2):
+            for j in (2, 0, 1):
+                project(hh - 3 + half, j)
         turn_supports(hh)
         quantise_relation(hh - 1)
         quantise_nodes(hh - 1)

@@ -17,13 +17,14 @@ STEPS = IT * GROUPS
 HALVES = STEPS // 2
 PREFETCH = 5
 TENSOR_A = 0
+WEIGHT_A = 1
 SCALAR_A = 1
 W0 = 4
 VECTOR_EXITS = 63
 FIRST_PROJECT = 13
 PROJECT_LAG = 9
 TURN_LAG = 5
-SCALAR_STEPS = tuple(range(4, 11)) + tuple(range(12, 32, 2))
+SCALAR_STEPS = (5, 7, 9, 11) + tuple(range(15, 30, 6))
 
 F32 = mybir.dt.float32
 BF16 = mybir.dt.bfloat16
@@ -41,6 +42,14 @@ def on_tensor(s, a):
     return a == TENSOR_A and s % 2 == 0 and s < STEPS - 2
 
 
+def on_weights(s, a):
+    return a == WEIGHT_A and s % 2 == 0 and 2 <= s < STEPS - 2
+
+
+def unsorted(s, a):
+    return on_tensor(s, a) or on_weights(s, a)
+
+
 def on_scalar(s, a):
     return (a == SCALAR_A and s in SCALAR_STEPS) or (s, a) == (1, 2)
 
@@ -56,7 +65,6 @@ def tile_relationalgraphconvolution_pa_kernel(
         work = ctx.enter_context(tc.tile_pool(name="work", bufs=2))
         three = ctx.enter_context(tc.tile_pool(name="three", bufs=3))
         four = ctx.enter_context(tc.tile_pool(name="four", bufs=4))
-        late = ctx.enter_context(tc.tile_pool(name="late", bufs=7))
         ring = ctx.enter_context(tc.psum_pool(name="ring", bufs=7))
         sump = ctx.enter_context(tc.psum_pool(name="sump", bufs=1))
         ctx.enter_context(tc.manual_schedule())
@@ -69,6 +77,8 @@ def tile_relationalgraphconvolution_pa_kernel(
         m0 = TENSOR_A * 16
         nc.vector.memset(mask[:], 0.0)
         nc.vector.memset(mask[:, m0 : m0 + 16], 1.0)
+        ones = keep.tile([P, 1], BF16, name="ones", align_bytes=64)
+        nc.vector.memset(ones[:], 1.0)
         nf_raw = keep.tile([P, 4, 4 * DE], BF16, name="nf_raw", align_bytes=64)
         nf_grp = keep.tile([P, 4 * 4 * DE], BF16, name="nf_grp", align_bytes=64)
         nf_codes = keep.tile([P, 4 * DE], U32, name="nf_codes", align_bytes=64)
@@ -162,7 +172,7 @@ def tile_relationalgraphconvolution_pa_kernel(
             for c in range(2):
                 for u in range(2):
                     k0 = (c * 2 + u) * P
-                    if on_tensor(s, a):
+                    if unsorted(s, a):
                         src = raw[s][:, a, :].bitcast(F32)[:, c * 256 + u : (c + 1) * 256 : 2]
                     else:
                         w0 = u * 256 + c * P
@@ -193,7 +203,7 @@ def tile_relationalgraphconvolution_pa_kernel(
             for a in range(a0, a0 + n):
                 for c in range(2):
                     cols = slice(a * 256 + c * P, a * 256 + (c + 1) * P)
-                    f0 = (c + 2) * DE if on_tensor(s, a) else c * DE
+                    f0 = (c + 2) * DE if unsorted(s, a) else c * DE
                     nc.tensor.matmul_mx(
                         out=mx[s][:, a * DE : (a + 1) * DE],
                         lhsT=codes[s][:, cols].bitcast(FP8X4),
@@ -215,8 +225,9 @@ def tile_relationalgraphconvolution_pa_kernel(
             )
 
         def turn_supports(hh, g0=0, n=2, copy=nc.scalar.copy):
-            if g0 == 0:
-                sgn[hh] = work.tile([P, 1024], BF16, name="sgn", align_bytes=64)
+            it, q0 = hh // 2, 2 * (hh % 2) + g0
+            if q0 == 0:
+                sgn[it] = work.tile([P, 2048], BF16, name="sgn", align_bytes=64)
             bank = ring.tile([P, 512], F32, name="bank")
             for b in range(n):
                 for u in range(2):
@@ -224,7 +235,7 @@ def tile_relationalgraphconvolution_pa_kernel(
                     w0 = (g0 + b) * 256 + u * P
                     nc.tensor.transpose(bank[:, k0 : k0 + P], supn[hh][:].bitcast(F32)[:, w0 : w0 + P], ident[:])
             copy(
-                out=sgn[hh][:, g0 * 512 : (g0 + n) * 512]
+                out=sgn[it][:, q0 * 512 : (q0 + n) * 512]
                 .bitcast(F32)
                 .rearrange("p (b i u) -> p b i u", b=n, u=2),
                 in_=bank[:, 0 : n * 256].rearrange("p (b u i) -> p b i u", b=n, u=2),
@@ -255,6 +266,21 @@ def tile_relationalgraphconvolution_pa_kernel(
                     stop=False,
                 )
 
+        def weight_sum(s):
+            bank = ring.tile([P, 512], F32, name="bank")
+            for c in range(2):
+                c0 = WEIGHT_A * N + c * 512
+                for t in range(4):
+                    nc.tensor.matmul(
+                        bank[:, 0:1],
+                        lhsT=grp[s][:, c0 + t : c0 + 512 : 4],
+                        rhs=ones[:],
+                        start=(c == 0 and t == 0),
+                        stop=(c == 1 and t == 3),
+                    )
+            col = s * RG + WEIGHT_A
+            nc.scalar.copy(out=rs[:, col : col + 1], in_=bank[:, 0:1])
+
         def turn_sums(hh):
             if on_tensor(2 * hh, TENSOR_A):
                 nc.tensor.matmul(
@@ -273,46 +299,45 @@ def tile_relationalgraphconvolution_pa_kernel(
                 op=ADD,
             )
 
-        def relation_part(hh, src, engine, i0=0, n=P):
-            if i0 == 0:
-                sgr[hh] = work.tile([P, 512], BF16, name="sgr", align_bytes=64)
+        def relation_part(hh, src, engine):
+            it, h = hh // 2, hh % 2
+            if h == 0:
+                sgr[it] = work.tile([P, 1024], BF16, name="sgr", align_bytes=64)
             engine.tensor_tensor(
-                out=sgr[hh][:, i0 * 4 : (i0 + n) * 4].rearrange("p (i t) -> p i t", t=4),
-                in0=src[:, i0 : i0 + n].unsqueeze(2).to_broadcast([P, n, 4]),
-                in1=relf[:, hh % 2, :].unsqueeze(1).to_broadcast([P, n, 4]),
+                out=sgr[it][:, h * 512 : (h + 1) * 512].rearrange("p (i t) -> p i t", t=4),
+                in0=src[:, 0:P].unsqueeze(2).to_broadcast([P, P, 4]),
+                in1=relf[:, h, :].unsqueeze(1).to_broadcast([P, P, 4]),
                 op=MULT,
             )
 
-        def quantise_relation(hh):
-            scodes[hh] = late.tile([P, 3 * P], U32, name="scodes", align_bytes=64)
-            sscales[hh] = late.tile([P, 3 * P], U8, name="sscales", align_bytes=64)
+        def quantise_relation(it):
+            scodes[it] = three.tile([P, 6 * P], U32, name="scodes", align_bytes=64)
+            sscales[it] = three.tile([P, 6 * P], U8, name="sscales", align_bytes=64)
             nc.vector.quantize_mx(
-                out=scodes[hh][:, 2 * P : 3 * P].bitcast(FP8X4), scales=sscales[hh][:, 2 * P : 3 * P], in_=sgr[hh][:]
+                out=scodes[it][:, 4 * P : 6 * P].bitcast(FP8X4), scales=sscales[it][:, 4 * P : 6 * P], in_=sgr[it][:]
             )
 
-        def quantise_nodes(hh, g0=0, n=2):
-            cols = slice(g0 * P, (g0 + n) * P)
+        def quantise_nodes(it, q0=0, n=4):
+            cols = slice(q0 * P, (q0 + n) * P)
             nc.vector.quantize_mx(
-                out=scodes[hh][:, cols].bitcast(FP8X4),
-                scales=sscales[hh][:, cols],
-                in_=sgn[hh][:, g0 * 512 : (g0 + n) * 512],
+                out=scodes[it][:, cols].bitcast(FP8X4),
+                scales=sscales[it][:, cols],
+                in_=sgn[it][:, q0 * 512 : (q0 + n) * 512],
             )
 
-        def project(hh, j):
-            it, h = hh // 2, hh % 2
-            first = h == 0 and j == 2
-            if first:
-                obank[it] = ring.tile([P, 512], F32, name="bank")
-            q = 4 + h if j == 2 else 2 * h + j
-            nc.tensor.matmul_mx(
-                out=obank[it][:, 0:NB],
-                lhsT=scodes[hh][:, j * P : (j + 1) * P].bitcast(FP8X4),
-                lhsT_scale=sscales[hh][:, j * P : (j + 1) * P],
-                rhs=w_codes[:, q * NB : (q + 1) * NB].bitcast(FP8X4),
-                rhs_scale=w_scales[:, q * NB : (q + 1) * NB],
-                start=first,
-                stop=(h == 1 and j == 1),
-            )
+        def project(it, passes):
+            for q in passes:
+                if q == 4:
+                    obank[it] = ring.tile([P, 512], F32, name="bank")
+                nc.tensor.matmul_mx(
+                    out=obank[it][:, 0:NB],
+                    lhsT=scodes[it][:, q * P : (q + 1) * P].bitcast(FP8X4),
+                    lhsT_scale=sscales[it][:, q * P : (q + 1) * P],
+                    rhs=w_codes[:, q * NB : (q + 1) * NB].bitcast(FP8X4),
+                    rhs_scale=w_scales[:, q * NB : (q + 1) * NB],
+                    start=(q == 4),
+                    stop=(q == 3),
+                )
 
         def store(it):
             res = work.tile([P, NB], F32, name="res", align_bytes=64)
@@ -350,25 +375,17 @@ def tile_relationalgraphconvolution_pa_kernel(
             )
 
         load(0, 4)
-        load_features()
         load(1, 2)
         load(2, 2)
+        load_features()
+        load(3, 2)
         nc.sync.dma_start(out=relf[:], in_=relation_features[0].rearrange("(h r) (q t) -> (r q) h t", h=2, t=4))
-        for s in range(3, PREFETCH):
+        for s in range(4, PREFETCH):
             load(s)
 
         for col in range(2 * RG - 1):
-            if not on_tensor(col // RG, col % RG) and not on_scalar(col // RG, col % RG):
+            if not unsorted(col // RG, col % RG) and not on_scalar(col // RG, col % RG):
                 row_sum(col // RG, col % RG)
-
-        nc.gpsimd.tensor_scalar(
-            out=nf_grp[:].rearrange("p (c d t) -> p c d t", c=4, t=4),
-            in0=nf_raw[:].rearrange("p c (t d) -> p c d t", t=4),
-            scalar1=1.0,
-            scalar2=0.0,
-            op0=MULT,
-            op1=ADD,
-        )
 
         pair_order = (2, 0, 1)
         project_at = {max(4 * it + PROJECT_LAG, 2 * it + FIRST_PROJECT): it for it in range(IT)}
@@ -378,14 +395,14 @@ def tile_relationalgraphconvolution_pa_kernel(
                 load(s + PREFETCH)
             if s < 3:
                 load_weights(pair_order[s])
-            if s == 1:
+            if s == 2:
                 nc.vector.quantize_mx(out=nf_codes[:].bitcast(FP8X4), scales=nf_scales[:], in_=nf_grp[:])
-            if s >= 2:
+            if s >= 3:
                 quantise(s - 1)
-            if s >= 4 and s % 2 == 0:
-                quantise_relation((s - 4) // 2)
-            if s >= TURN_LAG + 1 and (s - TURN_LAG) % 2 == 1:
-                quantise_nodes((s - TURN_LAG - 1) // 2)
+            if s >= 6 and s % 4 == 2:
+                quantise_relation((s - 6) // 4)
+            if s >= 8 and s % 4 == 0:
+                quantise_nodes((s - 8) // 4)
             if W0 + 4 <= s < W0 + 10 and (s - W0) % 2 == 0:
                 quantise_weights(pair_order[(s - W0 - 4) // 2])
             if W0 <= s < W0 + 6:
@@ -403,59 +420,60 @@ def tile_relationalgraphconvolution_pa_kernel(
                 turn_supports((s - TURN_LAG) // 2)
             if s == 0:
                 row_sum(1, 2)
+            if s == 1:
+                for v in range(2):
+                    nc.scalar.copy(
+                        out=nf_grp[:, v * 1024 : (v + 1) * 1024].rearrange("p (c d t) -> p c d t", c=2, t=4),
+                        in_=nf_raw[:, 2 * v : 2 * v + 2, :].rearrange("p c (t d) -> p c d t", t=4),
+                    )
             if s >= 2 and s % 2 == 0 and on_tensor(s - 2, TENSOR_A):
                 for c in range(2):
                     tensor_sum((s - 2) // 2, c)
+            if on_weights(s - 1, WEIGHT_A):
+                weight_sum(s - 1)
             if s >= 2:
                 aggregate(s - 2, 0, RG)
             if s in project_at:
-                for half in range(2):
-                    for j in (2, 0, 1):
-                        project(2 * project_at[s] + half, j)
+                project(project_at[s], (4, 5, 0, 1, 2, 3))
             if s >= 2:
                 keep_supports(s - 2)
             if s in project_at:
                 store(project_at[s])
-            if s >= 3 and s % 2 == 1:
+            if 3 <= s < STEPS - 1 and s % 2 == 1:
                 hh = (s - 3) // 2
                 collect_sums(hh)
-                if s + 1 < STEPS:
-                    relation_part(hh, sums[hh], nc.gpsimd)
+                relation_part(hh, sums[hh], nc.gpsimd)
             if s + 1 < STEPS:
-                if s % 2 == 1:
-                    row_sum(s + 1, RG - 2)
                 row_sum(s + 1, RG - 1)
-                if s % 2 == 0:
-                    spread_sums(s // 2)
-            if s == 0:
-                quantise(0)
+                if s % 2 == 0 and s >= 2:
+                    spread_sums((s - 2) // 2)
+            if s < 2:
+                quantise(s)
             if s + 2 < STEPS:
-                for a in range(RG - 2 + s % 2):
-                    if not on_tensor(s + 2, a) and not on_scalar(s + 2, a):
+                for a in range(RG - 1):
+                    if not unsorted(s + 2, a) and not on_scalar(s + 2, a):
                         row_sum(s + 2, a)
 
-        s, hh = STEPS - 1, HALVES - 1
-        turn_sums(hh)
+        s, hh, it = STEPS - 1, HALVES - 1, IT - 1
+        spread_sums(hh)
         aggregate(s - 1, 0, RG)
         quantise(s, 0, 2)
-        relation_part(hh - 1, sums[hh - 1], nc.vector)
         quantise(s, 2, 2)
+        collect_sums(hh - 1)
         keep_supports(s - 1)
-        aggregate(s, 0, RG)
         turn_supports(hh - 1)
-        quantise_nodes(hh - 2)
+        turn_sums(hh)
+        aggregate(s, 0, RG)
+        keep_supports(s)
+        quantise_nodes(it - 1)
+        relation_part(hh - 1, sums[hh - 1], nc.vector)
         relation_part(hh, sbank[hh], nc.vector)
-        keep_supports(s, copy=nc.vector.tensor_copy)
-        for half in range(2):
-            for j in (2, 0, 1):
-                project(hh - 3 + half, j)
+        quantise_relation(it)
+        quantise_nodes(it, 0, 2)
         turn_supports(hh)
-        quantise_relation(hh - 1)
-        quantise_nodes(hh - 1)
-        quantise_relation(hh)
-        store(IT - 2)
-        quantise_nodes(hh)
-        for half in range(2):
-            for j in (2, 0, 1):
-                project(hh - 1 + half, j)
-        store(IT - 1)
+        project(it - 1, (4, 5, 0, 1, 2, 3))
+        project(it, (4, 5, 0, 1))
+        store(it - 1)
+        quantise_nodes(it, 2, 2)
+        project(it, (2, 3))
+        store(it)

@@ -20,11 +20,11 @@ TENSOR_A = 0
 WEIGHT_A = 1
 SCALAR_A = 1
 W0 = 4
-VECTOR_EXITS = 63
+VECTOR_EXITS = 64
 FIRST_PROJECT = 13
 PROJECT_LAG = 9
 TURN_LAG = 5
-SCALAR_STEPS = (5, 7, 9, 11) + tuple(range(15, 30, 6))
+SCALAR_STEPS = (5, 7, 9, 11) + tuple(range(15, 32, 4))
 
 F32 = mybir.dt.float32
 BF16 = mybir.dt.bfloat16
@@ -72,7 +72,9 @@ def tile_relationalgraphconvolution_pa_kernel(
         ident = keep.tile([P, P], F32, name="ident", align_bytes=64)
         make_identity(nc, ident[:])
         rs = keep.tile([P, IT * R], F32, name="rs", align_bytes=64)
-        nc.vector.memset(rs[:], 0.0)
+        rep = [keep.tile([P, P], F32, name="rep%d" % h, align_bytes=64) for h in range(2)]
+        for h in range(2):
+            nc.vector.memset(rep[h][:, TENSOR_A * 16 : (TENSOR_A + 1) * 16], 0.0)
         mask = keep.tile([P, P], BF16, name="mask", align_bytes=64)
         m0 = TENSOR_A * 16
         nc.vector.memset(mask[:], 0.0)
@@ -97,7 +99,6 @@ def tile_relationalgraphconvolution_pa_kernel(
         codes = {}
         scales = {}
         mx = {}
-        rep = {}
         sbank = {}
         sums = {}
         supn = {}
@@ -106,6 +107,7 @@ def tile_relationalgraphconvolution_pa_kernel(
         scodes = {}
         sscales = {}
         obank = {}
+        wbank = {}
 
         def load(s, pieces=1):
             it, g = s // GROUPS, s % GROUPS
@@ -242,10 +244,11 @@ def tile_relationalgraphconvolution_pa_kernel(
             )
 
         def spread_sums(hh):
-            rep[hh] = work.tile([P, P], F32, name="rep", align_bytes=64)
-            nc.gpsimd.tensor_scalar(
-                out=rep[hh][:].rearrange("p (r q) -> p r q", q=16),
-                in0=rs[:, hh * 8 : (hh + 1) * 8].unsqueeze(2).to_broadcast([P, 8, 16]),
+            r0 = sum(unsorted(2 * hh, a) for a in range(RG))
+            engine = nc.gpsimd if hh < HALVES - 1 else nc.vector
+            engine.tensor_scalar(
+                out=rep[hh % 2][:, r0 * 16 :].rearrange("p (r q) -> p r q", q=16),
+                in0=rs[:, hh * 8 + r0 : (hh + 1) * 8].unsqueeze(2).to_broadcast([P, 8 - r0, 16]),
                 scalar1=1.0,
                 scalar2=0.0,
                 op0=MULT,
@@ -266,29 +269,33 @@ def tile_relationalgraphconvolution_pa_kernel(
                     stop=False,
                 )
 
-        def weight_sum(s):
-            bank = ring.tile([P, 512], F32, name="bank")
-            for c in range(2):
-                c0 = WEIGHT_A * N + c * 512
-                for t in range(4):
-                    nc.tensor.matmul(
-                        bank[:, 0:1],
-                        lhsT=grp[s][:, c0 + t : c0 + 512 : 4],
-                        rhs=ones[:],
-                        start=(c == 0 and t == 0),
-                        stop=(c == 1 and t == 3),
-                    )
-            col = s * RG + WEIGHT_A
-            nc.scalar.copy(out=rs[:, col : col + 1], in_=bank[:, 0:1])
+        def weight_sum(s, c):
+            if c == 0:
+                wbank[s] = ring.tile([P, 512], F32, name="bank")
+            c0 = WEIGHT_A * N + c * 512
+            for t in range(4):
+                nc.tensor.matmul(
+                    wbank[s][:, 0:1],
+                    lhsT=grp[s][:, c0 + t : c0 + 512 : 4],
+                    rhs=ones[:],
+                    start=(c == 0 and t == 0),
+                    stop=(c == 1 and t == 3),
+                )
+
+        def keep_sum(s):
+            nc.scalar.copy(
+                out=rep[s // 2 % 2][:, WEIGHT_A * 16 : (WEIGHT_A + 1) * 16],
+                in_=wbank[s][:, 0:1].to_broadcast([P, 16]),
+            )
 
         def turn_sums(hh):
             if on_tensor(2 * hh, TENSOR_A):
                 nc.tensor.matmul(
-                    sbank[hh][:, 0:256:2], lhsT=rep[hh][:], rhs=ident[:], start=False, stop=True, is_transpose=True
+                    sbank[hh][:, 0:256:2], lhsT=rep[hh % 2][:], rhs=ident[:], start=False, stop=True, is_transpose=True
                 )
             else:
                 sbank[hh] = sump.tile([P, 256], F32, name="sb")
-                nc.tensor.transpose(sbank[hh][:, 0:P], rep[hh][:], ident[:])
+                nc.tensor.transpose(sbank[hh][:, 0:P], rep[hh % 2][:], ident[:])
 
         def collect_sums(hh):
             sums[hh] = work.tile([P, P], F32, name="sums", align_bytes=64)
@@ -388,7 +395,7 @@ def tile_relationalgraphconvolution_pa_kernel(
                 row_sum(col // RG, col % RG)
 
         pair_order = (2, 0, 1)
-        project_at = {max(4 * it + PROJECT_LAG, 2 * it + FIRST_PROJECT): it for it in range(IT)}
+        project_at = {max(4 * it + PROJECT_LAG, it + FIRST_PROJECT): it for it in range(IT)}
 
         for s in range(STEPS):
             if s + PREFETCH < STEPS:
@@ -430,13 +437,17 @@ def tile_relationalgraphconvolution_pa_kernel(
                 for c in range(2):
                     tensor_sum((s - 2) // 2, c)
             if on_weights(s - 1, WEIGHT_A):
-                weight_sum(s - 1)
+                weight_sum(s - 1, 0)
             if s >= 2:
                 aggregate(s - 2, 0, RG)
+            if on_weights(s - 1, WEIGHT_A):
+                weight_sum(s - 1, 1)
             if s in project_at:
                 project(project_at[s], (4, 5, 0, 1, 2, 3))
             if s >= 2:
                 keep_supports(s - 2)
+            if on_weights(s - 1, WEIGHT_A):
+                keep_sum(s - 1)
             if s in project_at:
                 store(project_at[s])
             if 3 <= s < STEPS - 1 and s % 2 == 1:
@@ -445,8 +456,8 @@ def tile_relationalgraphconvolution_pa_kernel(
                 relation_part(hh, sums[hh], nc.gpsimd)
             if s + 1 < STEPS:
                 row_sum(s + 1, RG - 1)
-                if s % 2 == 0 and s >= 2:
-                    spread_sums((s - 2) // 2)
+                if s % 2 == 0:
+                    spread_sums(s // 2)
             if s < 2:
                 quantise(s)
             if s + 2 < STEPS:
@@ -455,25 +466,24 @@ def tile_relationalgraphconvolution_pa_kernel(
                         row_sum(s + 2, a)
 
         s, hh, it = STEPS - 1, HALVES - 1, IT - 1
-        spread_sums(hh)
         aggregate(s - 1, 0, RG)
         quantise(s, 0, 2)
-        quantise(s, 2, 2)
         collect_sums(hh - 1)
+        quantise(s, 2, 2)
+        quantise_nodes(it - 1)
         keep_supports(s - 1)
-        turn_supports(hh - 1)
         turn_sums(hh)
         aggregate(s, 0, RG)
         keep_supports(s)
-        quantise_nodes(it - 1)
+        turn_supports(hh - 1)
+        turn_supports(hh)
+        project(it - 1, (4, 5, 0, 1, 2, 3))
+        store(it - 1)
         relation_part(hh - 1, sums[hh - 1], nc.vector)
         relation_part(hh, sbank[hh], nc.vector)
         quantise_relation(it)
         quantise_nodes(it, 0, 2)
-        turn_supports(hh)
-        project(it - 1, (4, 5, 0, 1, 2, 3))
         project(it, (4, 5, 0, 1))
-        store(it - 1)
         quantise_nodes(it, 2, 2)
         project(it, (2, 3))
         store(it)

@@ -18,13 +18,15 @@ HALVES = STEPS // 2
 PREFETCH = 5
 TENSOR_A = 0
 WEIGHT_A = 1
+SECOND_A = 1
+SECOND = (6, 8)
 SCALAR_A = 1
 W0 = 4
 VECTOR_EXITS = 64
 FIRST_PROJECT = 13
 PROJECT_LAG = 9
 TURN_LAG = 5
-SCALAR_STEPS = (5, 7, 9, 11) + tuple(range(15, 32, 4))
+SCALAR_STEPS = (5, 7, 9, 11) + tuple(range(13, 32, 4))
 
 F32 = mybir.dt.float32
 BF16 = mybir.dt.bfloat16
@@ -39,11 +41,11 @@ FLOPS = 2 * (R * N * N * DE + N * R * F * NB)
 
 
 def on_tensor(s, a):
-    return a == TENSOR_A and s % 2 == 0 and s < STEPS - 2
+    return (a == TENSOR_A and s % 2 == 0 and s < STEPS - 2) or (a == SECOND_A and s in SECOND)
 
 
 def on_weights(s, a):
-    return a == WEIGHT_A and s % 2 == 0 and 2 <= s < STEPS - 2
+    return a == WEIGHT_A and s % 2 == 0 and 2 <= s < STEPS - 2 and not on_tensor(s, a)
 
 
 def unsorted(s, a):
@@ -75,10 +77,12 @@ def tile_relationalgraphconvolution_pa_kernel(
         rep = [keep.tile([P, P], F32, name="rep%d" % h, align_bytes=64) for h in range(2)]
         for h in range(2):
             nc.vector.memset(rep[h][:, TENSOR_A * 16 : (TENSOR_A + 1) * 16], 0.0)
-        mask = keep.tile([P, P], BF16, name="mask", align_bytes=64)
-        m0 = TENSOR_A * 16
+        mask = keep.tile([P, 2, P], BF16, name="mask", align_bytes=64)
         nc.vector.memset(mask[:], 0.0)
-        nc.vector.memset(mask[:, m0 : m0 + 16], 1.0)
+        for j, a in enumerate((TENSOR_A, SECOND_A)):
+            nc.vector.memset(mask[:, j, a * 16 : (a + 1) * 16], 1.0)
+        for s in SECOND:
+            nc.vector.memset(rs[:, s * RG + SECOND_A : s * RG + SECOND_A + 1], 0.0)
         ones = keep.tile([P, 1], BF16, name="ones", align_bytes=64)
         nc.vector.memset(ones[:], 1.0)
         nf_raw = keep.tile([P, 4, 4 * DE], BF16, name="nf_raw", align_bytes=64)
@@ -244,7 +248,7 @@ def tile_relationalgraphconvolution_pa_kernel(
             )
 
         def spread_sums(hh):
-            r0 = sum(unsorted(2 * hh, a) for a in range(RG))
+            r0 = on_tensor(2 * hh, TENSOR_A) + on_weights(2 * hh, WEIGHT_A)
             engine = nc.gpsimd if hh < HALVES - 1 else nc.vector
             engine.tensor_scalar(
                 out=rep[hh % 2][:, r0 * 16 :].rearrange("p (r q) -> p r q", q=16),
@@ -255,19 +259,20 @@ def tile_relationalgraphconvolution_pa_kernel(
                 op1=ADD,
             )
 
-        def tensor_sum(hh, c):
-            if c == 0:
+        def tensor_sum(hh, j, a):
+            if j == 0:
                 sbank[hh] = sump.tile([P, 256], F32, name="sb")
-            c0 = TENSOR_A * N + c * 512
-            words = grp[2 * hh][:, c0 : c0 + 512].rearrange("p (i u e) -> p u i e", u=2, e=2)
-            for u in range(2):
-                nc.tensor.matmul(
-                    sbank[hh][:].rearrange("p (i e) -> p i e", e=2),
-                    lhsT=mask[:],
-                    rhs=words[:, u],
-                    start=(c == 0 and u == 0),
-                    stop=False,
-                )
+            for c in range(2):
+                c0 = a * N + c * 512
+                words = grp[2 * hh][:, c0 : c0 + 512].rearrange("p (i u e) -> p u i e", u=2, e=2)
+                for u in range(2):
+                    nc.tensor.matmul(
+                        sbank[hh][:].rearrange("p (i e) -> p i e", e=2),
+                        lhsT=mask[:, j, :],
+                        rhs=words[:, u],
+                        start=(j == 0 and c == 0 and u == 0),
+                        stop=False,
+                    )
 
         def weight_sum(s, c):
             if c == 0:
@@ -433,9 +438,9 @@ def tile_relationalgraphconvolution_pa_kernel(
                         out=nf_grp[:, v * 1024 : (v + 1) * 1024].rearrange("p (c d t) -> p c d t", c=2, t=4),
                         in_=nf_raw[:, 2 * v : 2 * v + 2, :].rearrange("p c (t d) -> p c d t", t=4),
                     )
-            if s >= 2 and s % 2 == 0 and on_tensor(s - 2, TENSOR_A):
-                for c in range(2):
-                    tensor_sum((s - 2) // 2, c)
+            for j, a in enumerate((TENSOR_A, SECOND_A)):
+                if s >= 2 and on_tensor(s - 2, a):
+                    tensor_sum((s - 2) // 2, j, a)
             if on_weights(s - 1, WEIGHT_A):
                 weight_sum(s - 1, 0)
             if s >= 2:

@@ -18,15 +18,16 @@ HALVES = STEPS // 2
 PREFETCH = 5
 TENSOR_A = 0
 WEIGHT_A = 1
-SECOND_A = 1
+SECOND_A = 2
 SECOND = (6, 8)
+DOUBLE = (16, 20, 24, 28)
 SCALAR_A = 1
 W0 = 4
 VECTOR_EXITS = 64
 FIRST_PROJECT = 13
 PROJECT_LAG = 9
 TURN_LAG = 5
-SCALAR_STEPS = (5, 7, 9, 11) + tuple(range(13, 32, 4))
+SCALAR_STEPS = (5, 7, 11) + tuple(range(15, 32, 8))
 
 F32 = mybir.dt.float32
 BF16 = mybir.dt.bfloat16
@@ -45,7 +46,7 @@ def on_tensor(s, a):
 
 
 def on_weights(s, a):
-    return a == WEIGHT_A and s % 2 == 0 and 2 <= s < STEPS - 2 and not on_tensor(s, a)
+    return (a == WEIGHT_A and s % 2 == 0 and 2 <= s < STEPS - 2) or (a == WEIGHT_A + 1 and s in DOUBLE)
 
 
 def unsorted(s, a):
@@ -248,7 +249,7 @@ def tile_relationalgraphconvolution_pa_kernel(
             )
 
         def spread_sums(hh):
-            r0 = on_tensor(2 * hh, TENSOR_A) + on_weights(2 * hh, WEIGHT_A)
+            r0 = on_tensor(2 * hh, TENSOR_A) + sum(on_weights(2 * hh, a) for a in range(RG))
             engine = nc.gpsimd if hh < HALVES - 1 else nc.vector
             engine.tensor_scalar(
                 out=rep[hh % 2][:, r0 * 16 :].rearrange("p (r q) -> p r q", q=16),
@@ -274,23 +275,23 @@ def tile_relationalgraphconvolution_pa_kernel(
                         stop=False,
                     )
 
-        def weight_sum(s, c):
-            if c == 0:
+        def weight_sum(s, j, last):
+            if j == 0:
                 wbank[s] = ring.tile([P, 512], F32, name="bank")
-            c0 = WEIGHT_A * N + c * 512
+            c0 = WEIGHT_A * N + j * 512
             for t in range(4):
                 nc.tensor.matmul(
-                    wbank[s][:, 0:1],
+                    wbank[s][:, j // 2 : j // 2 + 1],
                     lhsT=grp[s][:, c0 + t : c0 + 512 : 4],
                     rhs=ones[:],
-                    start=(c == 0 and t == 0),
-                    stop=(c == 1 and t == 3),
+                    start=(j == 0 and t == 0),
+                    stop=(last and t == 3),
                 )
 
-        def keep_sum(s):
+        def keep_sums(s, n):
             nc.scalar.copy(
-                out=rep[s // 2 % 2][:, WEIGHT_A * 16 : (WEIGHT_A + 1) * 16],
-                in_=wbank[s][:, 0:1].to_broadcast([P, 16]),
+                out=rep[s // 2 % 2][:, WEIGHT_A * 16 : (WEIGHT_A + n) * 16].rearrange("p (r q) -> p r q", q=16),
+                in_=wbank[s][:, 0:n].unsqueeze(2).to_broadcast([P, n, 16]),
             )
 
         def turn_sums(hh):
@@ -441,18 +442,27 @@ def tile_relationalgraphconvolution_pa_kernel(
             for j, a in enumerate((TENSOR_A, SECOND_A)):
                 if s >= 2 and on_tensor(s - 2, a):
                     tensor_sum((s - 2) // 2, j, a)
-            if on_weights(s - 1, WEIGHT_A):
-                weight_sum(s - 1, 0)
-            if s >= 2:
-                aggregate(s - 2, 0, RG)
-            if on_weights(s - 1, WEIGHT_A):
-                weight_sum(s - 1, 1)
-            if s in project_at:
-                project(project_at[s], (4, 5, 0, 1, 2, 3))
+            tiles = sum(on_weights(s - 1, a) for a in range(RG))
+            if tiles == 2:
+                for j in range(2):
+                    weight_sum(s - 1, j, False)
+                    aggregate(s - 2, 2 * j, 2)
+                for j in range(2):
+                    weight_sum(s - 1, 2 + j, j == 1)
+                    project(project_at[s], ((4, 5, 0), (1, 2, 3))[j])
+            else:
+                if tiles:
+                    weight_sum(s - 1, 0, False)
+                if s >= 2:
+                    aggregate(s - 2, 0, RG)
+                if tiles:
+                    weight_sum(s - 1, 1, True)
+                if s in project_at:
+                    project(project_at[s], (4, 5, 0, 1, 2, 3))
             if s >= 2:
                 keep_supports(s - 2)
-            if on_weights(s - 1, WEIGHT_A):
-                keep_sum(s - 1)
+            if tiles:
+                keep_sums(s - 1, tiles)
             if s in project_at:
                 store(project_at[s])
             if 3 <= s < STEPS - 1 and s % 2 == 1:

@@ -15,19 +15,11 @@ RG = 4
 GROUPS = R // RG
 STEPS = IT * GROUPS
 HALVES = STEPS // 2
+SPREAD = DR // 4
 PREFETCH = 5
-TENSOR_A = 0
-WEIGHT_A = 1
-SECOND_A = 2
-SECOND = (6, 8)
-DOUBLE = (16, 20, 24, 28)
-SCALAR_A = 1
-W0 = 4
-VECTOR_EXITS = 64
-FIRST_PROJECT = 13
-PROJECT_LAG = 9
-TURN_LAG = 5
-SCALAR_STEPS = (5, 7, 11) + tuple(range(15, 32, 8))
+W0 = 2
+FIRST_PROJECT = W0 + 14
+PROJECT_LAG = 8
 
 F32 = mybir.dt.float32
 BF16 = mybir.dt.bfloat16
@@ -36,25 +28,8 @@ U8 = mybir.dt.uint8
 FP8 = mybir.dt.float8_e4m3fn
 FP8X4 = mybir.dt.float8_e4m3fn_x4
 MULT = mybir.AluOpType.mult
-ADD = mybir.AluOpType.add
 
 FLOPS = 2 * (R * N * N * DE + N * R * F * NB)
-
-
-def on_tensor(s, a):
-    return (a == TENSOR_A and s % 2 == 0 and s < STEPS - 2) or (a == SECOND_A and s in SECOND)
-
-
-def on_weights(s, a):
-    return (a == WEIGHT_A and s % 2 == 0 and 2 <= s < STEPS - 2) or (a == WEIGHT_A + 1 and s in DOUBLE)
-
-
-def unsorted(s, a):
-    return on_tensor(s, a) or on_weights(s, a)
-
-
-def on_scalar(s, a):
-    return (a == SCALAR_A and s in SCALAR_STEPS) or (s, a) == (1, 2)
 
 
 def tile_relationalgraphconvolution_pa_kernel(
@@ -64,32 +39,21 @@ def tile_relationalgraphconvolution_pa_kernel(
     with ExitStack() as ctx:
         keep = ctx.enter_context(tc.tile_pool(name="keep", bufs=1))
         rawp = ctx.enter_context(tc.tile_pool(name="rawp", bufs=PREFETCH + 1))
-        permp = ctx.enter_context(tc.tile_pool(name="permp", bufs=12))
         work = ctx.enter_context(tc.tile_pool(name="work", bufs=2))
         three = ctx.enter_context(tc.tile_pool(name="three", bufs=3))
         four = ctx.enter_context(tc.tile_pool(name="four", bufs=4))
-        ring = ctx.enter_context(tc.psum_pool(name="ring", bufs=7))
-        sump = ctx.enter_context(tc.psum_pool(name="sump", bufs=1))
+        ring = ctx.enter_context(tc.psum_pool(name="ring", bufs=8))
         ctx.enter_context(tc.manual_schedule())
 
         ident = keep.tile([P, P], F32, name="ident", align_bytes=64)
         make_identity(nc, ident[:])
-        rs = keep.tile([P, IT * R], F32, name="rs", align_bytes=64)
         rep = [keep.tile([P, P], F32, name="rep%d" % h, align_bytes=64) for h in range(2)]
-        for h in range(2):
-            nc.vector.memset(rep[h][:, TENSOR_A * 16 : (TENSOR_A + 1) * 16], 0.0)
-        mask = keep.tile([P, 2, P], BF16, name="mask", align_bytes=64)
-        nc.vector.memset(mask[:], 0.0)
-        for j, a in enumerate((TENSOR_A, SECOND_A)):
-            nc.vector.memset(mask[:, j, a * 16 : (a + 1) * 16], 1.0)
-        for s in SECOND:
-            nc.vector.memset(rs[:, s * RG + SECOND_A : s * RG + SECOND_A + 1], 0.0)
-        ones = keep.tile([P, 1], BF16, name="ones", align_bytes=64)
+        ones = keep.tile([P, SPREAD], BF16, name="ones", align_bytes=64)
         nc.vector.memset(ones[:], 1.0)
-        nf_raw = keep.tile([P, 4, 4 * DE], BF16, name="nf_raw", align_bytes=64)
-        nf_grp = keep.tile([P, 4 * 4 * DE], BF16, name="nf_grp", align_bytes=64)
-        nf_codes = keep.tile([P, 4 * DE], U32, name="nf_codes", align_bytes=64)
-        nf_scales = keep.tile([P, 4 * DE], U8, name="nf_scales", align_bytes=64)
+        nf_raw = keep.tile([P, 2, 4 * DE], BF16, name="nf_raw", align_bytes=64)
+        nf_grp = keep.tile([P, 2 * 4 * DE], BF16, name="nf_grp", align_bytes=64)
+        nf_codes = keep.tile([P, 2 * DE], U32, name="nf_codes", align_bytes=64)
+        nf_scales = keep.tile([P, 2 * DE], U8, name="nf_scales", align_bytes=64)
         relf = keep.tile([P, 2, 4], BF16, name="relf", align_bytes=64)
         w_bytes = keep.tile([P, 2 * R * F], U8, name="w_bytes", align_bytes=64)
         w_scale = keep.tile([P, R * F], F32, name="w_scale", align_bytes=64)
@@ -105,7 +69,6 @@ def tile_relationalgraphconvolution_pa_kernel(
         scales = {}
         mx = {}
         sbank = {}
-        sums = {}
         supn = {}
         sgn = {}
         sgr = {}
@@ -116,12 +79,12 @@ def tile_relationalgraphconvolution_pa_kernel(
 
         def load(s, pieces=1):
             it, g = s // GROUPS, s % GROUPS
-            raw[s] = rawp.tile([P, RG, N], BF16, name="raw", align_bytes=64)
+            raw[s] = rawp.tile([P, RG * N], BF16, name="raw", align_bytes=64)
             n = RG // pieces
             for a in range(pieces):
                 r0 = g * RG + a * n
                 nc.sync.dma_start(
-                    out=raw[s][:, a * n : (a + 1) * n, :],
+                    out=raw[s][:, a * n * N : (a + 1) * n * N].rearrange("p (r j) -> p r j", j=N),
                     in_=adj[0, r0 : r0 + n, it * P : (it + 1) * P, :].rearrange("r i j -> i r j"),
                 )
 
@@ -130,9 +93,6 @@ def tile_relationalgraphconvolution_pa_kernel(
             for c in range(2):
                 for u in range(2):
                     nc.sync.dma_start(out=nf_raw[:, c, u * 2 * DE : (u + 1) * 2 * DE], in_=runs[c, u])
-            nc.sync.dma_start(
-                out=nf_raw[:, 2:4, :], in_=node_features[0].rearrange("(c p t) d -> p c (t d)", p=P, t=4)
-            )
 
         def load_weights(pair):
             r0, n, f0, width = (0, R, DE, DR) if pair == 2 else (pair * 8, 8, 0, DE)
@@ -149,42 +109,28 @@ def tile_relationalgraphconvolution_pa_kernel(
                 in_=sc[r0 : r0 + n, f0 : f0 + width].partition_broadcast(P),
             )
 
-        def row_sum(s, a):
-            col = s * RG + a
-            perm[col] = permp.tile([P, N], BF16, name="perm", align_bytes=64)
-            dst = perm[col][:].rearrange("p (u q f) -> p u q f", u=2, f=16)
-            src = raw[s][:, a, :].rearrange("p (q u f) -> p u q f", u=2, f=16)
-            if on_scalar(s, a):
-                nc.scalar.activation(
-                    out=dst,
-                    in_=src,
-                    func=mybir.ActivationFunctionType.Copy,
-                    accum_out=rs[:, col : col + 1],
-                )
+        def sort(s, a0=0, n=RG):
+            if n == RG:
+                dst = three.tile([P, n * N], BF16, name="perm", align_bytes=64)
             else:
-                nc.vector.tensor_scalar(
-                    out=dst,
-                    in0=src,
-                    scalar1=1.0,
-                    scalar2=None,
-                    op0=MULT,
-                    op1=ADD,
-                    accum_out=rs[:, col : col + 1],
-                )
+                dst = four.tile([P, n * N], BF16, name="permpart", align_bytes=64)
+            for a in range(n):
+                perm[s, a0 + a] = (dst, n, a)
+            nc.vector.tensor_copy(
+                out=dst[:].rearrange("p (u q f) -> p u q f", u=2, f=16),
+                in_=raw[s][:, a0 * N : (a0 + n) * N].rearrange("p (q u f) -> p u q f", u=2, f=16),
+            )
 
         def turn(s, a):
             if a == 0:
-                grp[s] = four.tile([P, RG * N], BF16, name="grp", align_bytes=64)
+                grp[s] = three.tile([P, RG * N], BF16, name="grp", align_bytes=64)
+            src, n, al = perm[s, a]
             bank = ring.tile([P, 512], F32, name="bank")
             for c in range(2):
                 for u in range(2):
                     k0 = (c * 2 + u) * P
-                    if unsorted(s, a):
-                        src = raw[s][:, a, :].bitcast(F32)[:, c * 256 + u : (c + 1) * 256 : 2]
-                    else:
-                        w0 = u * 256 + c * P
-                        src = perm[s * RG + a][:].bitcast(F32)[:, w0 : w0 + P]
-                    nc.tensor.transpose(bank[:, k0 : k0 + P], src, ident[:])
+                    w0 = u * n * 256 + al * 256 + c * P
+                    nc.tensor.transpose(bank[:, k0 : k0 + P], src[:].bitcast(F32)[:, w0 : w0 + P], ident[:])
             return bank
 
         def empty(s, a, bank, copy=nc.scalar.copy):
@@ -204,143 +150,95 @@ def tile_relationalgraphconvolution_pa_kernel(
                 in_=grp[s][:, a0 * N : (a0 + n) * N],
             )
 
-        def aggregate(s, a0, n):
-            if a0 == 0:
-                mx[s] = ring.tile([P, 512], F32, name="bank")
-            for a in range(a0, a0 + n):
+        def aggregate(s):
+            mx[s] = ring.tile([P, 512], F32, name="bank")
+            for a in range(RG):
                 for c in range(2):
                     cols = slice(a * 256 + c * P, a * 256 + (c + 1) * P)
-                    f0 = (c + 2) * DE if unsorted(s, a) else c * DE
                     nc.tensor.matmul_mx(
                         out=mx[s][:, a * DE : (a + 1) * DE],
                         lhsT=codes[s][:, cols].bitcast(FP8X4),
                         lhsT_scale=scales[s][:, cols],
-                        rhs=nf_codes[:, f0 : f0 + DE].bitcast(FP8X4),
-                        rhs_scale=nf_scales[:, f0 : f0 + DE],
+                        rhs=nf_codes[:, c * DE : (c + 1) * DE].bitcast(FP8X4),
+                        rhs_scale=nf_scales[:, c * DE : (c + 1) * DE],
                         start=(c == 0),
                         stop=(c == 1),
                     )
 
-        def keep_supports(s, a0=0, n=RG, copy=nc.scalar.copy):
+        def keep_supports(s):
             hh, g = s // 2, s % 2
-            if g == 0 and a0 == 0:
+            if g == 0:
                 supn[hh] = three.tile([P, 1024], BF16, name="supn", align_bytes=64)
-            dst = supn[hh][:, g * 512 : (g + 1) * 512].rearrange("p (u q e) -> p u q e", u=2, e=2)
-            copy(
-                out=dst[:, :, a0 * 32 : (a0 + n) * 32, :],
-                in_=mx[s][:, a0 * DE : (a0 + n) * DE].rearrange("p (q u e) -> p u q e", u=2, e=2),
+            nc.scalar.copy(
+                out=supn[hh][:, g * 512 : (g + 1) * 512].rearrange("p (u q e) -> p u q e", u=2, e=2),
+                in_=mx[s][:].rearrange("p (q u e) -> p u q e", u=2, e=2),
             )
 
-        def turn_supports(hh, g0=0, n=2, copy=nc.scalar.copy):
-            it, q0 = hh // 2, 2 * (hh % 2) + g0
+        def turn_supports(hh):
+            it, q0 = hh // 2, 2 * (hh % 2)
             if q0 == 0:
                 sgn[it] = work.tile([P, 2048], BF16, name="sgn", align_bytes=64)
             bank = ring.tile([P, 512], F32, name="bank")
-            for b in range(n):
+            for b in range(2):
                 for u in range(2):
                     k0 = (b * 2 + u) * P
-                    w0 = (g0 + b) * 256 + u * P
-                    nc.tensor.transpose(bank[:, k0 : k0 + P], supn[hh][:].bitcast(F32)[:, w0 : w0 + P], ident[:])
-            copy(
-                out=sgn[it][:, q0 * 512 : (q0 + n) * 512]
-                .bitcast(F32)
-                .rearrange("p (b i u) -> p b i u", b=n, u=2),
-                in_=bank[:, 0 : n * 256].rearrange("p (b u i) -> p b i u", b=n, u=2),
+                    nc.tensor.transpose(bank[:, k0 : k0 + P], supn[hh][:].bitcast(F32)[:, k0 : k0 + P], ident[:])
+            nc.scalar.copy(
+                out=sgn[it][:, q0 * 512 : (q0 + 2) * 512].bitcast(F32).rearrange("p (b i u) -> p b i u", b=2, u=2),
+                in_=bank[:].rearrange("p (b u i) -> p b i u", b=2, u=2),
             )
 
-        def spread_sums(hh):
-            r0 = on_tensor(2 * hh, TENSOR_A) + sum(on_weights(2 * hh, a) for a in range(RG))
-            engine = nc.gpsimd if hh < HALVES - 1 else nc.vector
-            engine.tensor_scalar(
-                out=rep[hh % 2][:, r0 * 16 :].rearrange("p (r q) -> p r q", q=16),
-                in0=rs[:, hh * 8 + r0 : (hh + 1) * 8].unsqueeze(2).to_broadcast([P, 8 - r0, 16]),
-                scalar1=1.0,
-                scalar2=0.0,
-                op0=MULT,
-                op1=ADD,
-            )
-
-        def tensor_sum(hh, j, a):
-            if j == 0:
-                sbank[hh] = sump.tile([P, 256], F32, name="sb")
-            for c in range(2):
-                c0 = a * N + c * 512
-                words = grp[2 * hh][:, c0 : c0 + 512].rearrange("p (i u e) -> p u i e", u=2, e=2)
-                for u in range(2):
+        def row_sums(s):
+            wbank[s] = ring.tile([P, 512], F32, name="bank")
+            for a in range(RG):
+                for j in range(8):
+                    c0 = a * N + j // 4 * 512
                     nc.tensor.matmul(
-                        sbank[hh][:].rearrange("p (i e) -> p i e", e=2),
-                        lhsT=mask[:, j, :],
-                        rhs=words[:, u],
-                        start=(j == 0 and c == 0 and u == 0),
-                        stop=False,
+                        wbank[s][:, a * SPREAD : (a + 1) * SPREAD],
+                        lhsT=grp[s][:, c0 + j % 4 : c0 + 512 : 4],
+                        rhs=ones[:],
+                        start=(j == 0),
+                        stop=(j == 7),
                     )
 
-        def weight_sum(s, j, last):
-            if j == 0:
-                wbank[s] = ring.tile([P, 512], F32, name="bank")
-            c0 = WEIGHT_A * N + j * 512
-            for t in range(4):
-                nc.tensor.matmul(
-                    wbank[s][:, j // 2 : j // 2 + 1],
-                    lhsT=grp[s][:, c0 + t : c0 + 512 : 4],
-                    rhs=ones[:],
-                    start=(j == 0 and t == 0),
-                    stop=(last and t == 3),
-                )
-
-        def keep_sums(s, n):
-            nc.scalar.copy(
-                out=rep[s // 2 % 2][:, WEIGHT_A * 16 : (WEIGHT_A + n) * 16].rearrange("p (r q) -> p r q", q=16),
-                in_=wbank[s][:, 0:n].unsqueeze(2).to_broadcast([P, n, 16]),
-            )
+        def keep_sums(s):
+            nc.scalar.copy(out=rep[s // 2 % 2][:, s % 2 * 64 : s % 2 * 64 + 64], in_=wbank[s][:, 0:64])
 
         def turn_sums(hh):
-            if on_tensor(2 * hh, TENSOR_A):
-                nc.tensor.matmul(
-                    sbank[hh][:, 0:256:2], lhsT=rep[hh % 2][:], rhs=ident[:], start=False, stop=True, is_transpose=True
-                )
-            else:
-                sbank[hh] = sump.tile([P, 256], F32, name="sb")
-                nc.tensor.transpose(sbank[hh][:, 0:P], rep[hh % 2][:], ident[:])
+            sbank[hh] = ring.tile([P, 512], F32, name="bank")
+            nc.tensor.transpose(sbank[hh][:, 0:P], rep[hh % 2][:], ident[:])
 
-        def collect_sums(hh):
-            sums[hh] = work.tile([P, P], F32, name="sums", align_bytes=64)
-            nc.vector.tensor_reduce(
-                out=sums[hh][:],
-                in_=sbank[hh][:].rearrange("p (i e) -> p i e", e=2),
-                axis=mybir.AxisListType.X,
-                op=ADD,
-            )
-
-        def relation_part(hh, src, engine):
+        def relation_part(hh):
             it, h = hh // 2, hh % 2
             if h == 0:
                 sgr[it] = work.tile([P, 1024], BF16, name="sgr", align_bytes=64)
-            engine.tensor_tensor(
+            nc.vector.tensor_tensor(
                 out=sgr[it][:, h * 512 : (h + 1) * 512].rearrange("p (i t) -> p i t", t=4),
-                in0=src[:, 0:P].unsqueeze(2).to_broadcast([P, P, 4]),
+                in0=sbank[hh][:, 0:P].unsqueeze(2).to_broadcast([P, P, 4]),
                 in1=relf[:, h, :].unsqueeze(1).to_broadcast([P, P, 4]),
                 op=MULT,
             )
 
         def quantise_relation(it):
-            scodes[it] = three.tile([P, 6 * P], U32, name="scodes", align_bytes=64)
-            sscales[it] = three.tile([P, 6 * P], U8, name="sscales", align_bytes=64)
             nc.vector.quantize_mx(
                 out=scodes[it][:, 4 * P : 6 * P].bitcast(FP8X4), scales=sscales[it][:, 4 * P : 6 * P], in_=sgr[it][:]
             )
 
-        def quantise_nodes(it, q0=0, n=4):
-            cols = slice(q0 * P, (q0 + n) * P)
+        def quantise_nodes(hh):
+            it, q0 = hh // 2, 2 * (hh % 2)
+            if q0 == 0:
+                scodes[it] = four.tile([P, 6 * P], U32, name="scodes", align_bytes=64)
+                sscales[it] = four.tile([P, 6 * P], U8, name="sscales", align_bytes=64)
+            cols = slice(q0 * P, (q0 + 2) * P)
             nc.vector.quantize_mx(
                 out=scodes[it][:, cols].bitcast(FP8X4),
                 scales=sscales[it][:, cols],
-                in_=sgn[it][:, q0 * 512 : (q0 + n) * 512],
+                in_=sgn[it][:, q0 * 512 : (q0 + 2) * 512],
             )
 
         def project(it, passes):
             for q in passes:
-                if q == 4:
+                if q == 0:
                     obank[it] = ring.tile([P, 512], F32, name="bank")
                 nc.tensor.matmul_mx(
                     out=obank[it][:, 0:NB],
@@ -348,7 +246,7 @@ def tile_relationalgraphconvolution_pa_kernel(
                     lhsT_scale=sscales[it][:, q * P : (q + 1) * P],
                     rhs=w_codes[:, q * NB : (q + 1) * NB].bitcast(FP8X4),
                     rhs_scale=w_scales[:, q * NB : (q + 1) * NB],
-                    start=(q == 4),
+                    start=(q == 0),
                     stop=(q == 3),
                 )
 
@@ -387,118 +285,90 @@ def tile_relationalgraphconvolution_pa_kernel(
                 in_=w_grp[:, pair * 2048 : (pair + 1) * 2048],
             )
 
+        all_passes = (0, 1, 4, 5, 2, 3)
         load(0, 4)
-        load(1, 2)
-        load(2, 2)
         load_features()
-        load(3, 2)
+        load(1, 2)
         nc.sync.dma_start(out=relf[:], in_=relation_features[0].rearrange("(h r) (q t) -> (r q) h t", h=2, t=4))
-        for s in range(4, PREFETCH):
+        load(2)
+        load_weights(0)
+        for s in range(3, PREFETCH):
             load(s)
 
-        for col in range(2 * RG - 1):
-            if not unsorted(col // RG, col % RG) and not on_scalar(col // RG, col % RG):
-                row_sum(col // RG, col % RG)
-
-        pair_order = (2, 0, 1)
         project_at = {max(4 * it + PROJECT_LAG, it + FIRST_PROJECT): it for it in range(IT)}
 
         for s in range(STEPS):
+            w = s - W0
+            last = s == STEPS - 1
             if s + PREFETCH < STEPS:
                 load(s + PREFETCH)
-            if s < 3:
-                load_weights(pair_order[s])
-            if s == 2:
-                nc.vector.quantize_mx(out=nf_codes[:].bitcast(FP8X4), scales=nf_scales[:], in_=nf_grp[:])
-            if s >= 3:
-                quantise(s - 1)
-            if s >= 6 and s % 4 == 2:
-                quantise_relation((s - 6) // 4)
-            if s >= 8 and s % 4 == 0:
-                quantise_nodes((s - 8) // 4)
-            if W0 + 4 <= s < W0 + 10 and (s - W0) % 2 == 0:
-                quantise_weights(pair_order[(s - W0 - 4) // 2])
-            if W0 <= s < W0 + 6:
-                weight_values(pair_order[(s - W0) // 2], (s - W0) % 2)
-            if s >= 3 and s % 2 == 1:
-                turn_sums((s - 3) // 2)
+            if s in (0, 3):
+                load_weights(1 + s // 3)
+            if 1 <= s < STEPS - 1:
+                sort(s + 1)
             for a in range(RG):
-                to_vector = a % 2 == 1 and 2 * s + a // 2 >= VECTOR_EXITS
+                if s == 0:
+                    sort(0, a, 1)
+                if last:
+                    to_vector = a % 2 == 1
+                else:
+                    to_vector = a == 3 and s % 4 != 2 and not (0 <= w < 12 and w % 2 == 0)
                 empty(s, a, turn(s, a), nc.vector.tensor_copy if to_vector else nc.scalar.copy)
-                if a == 1 and s + 2 < STEPS and on_scalar(s + 2, SCALAR_A):
-                    row_sum(s + 2, SCALAR_A)
-            if W0 + 2 <= s < W0 + 8:
-                turn_weights(2 * pair_order[(s - W0 - 2) // 2] + (s - W0) % 2)
-            if s >= TURN_LAG and (s - TURN_LAG) % 2 == 0:
-                turn_supports((s - TURN_LAG) // 2)
             if s == 0:
-                row_sum(1, 2)
-            if s == 1:
-                for v in range(2):
-                    nc.scalar.copy(
-                        out=nf_grp[:, v * 1024 : (v + 1) * 1024].rearrange("p (c d t) -> p c d t", c=2, t=4),
-                        in_=nf_raw[:, 2 * v : 2 * v + 2, :].rearrange("p c (t d) -> p c d t", t=4),
-                    )
-            for j, a in enumerate((TENSOR_A, SECOND_A)):
-                if s >= 2 and on_tensor(s - 2, a):
-                    tensor_sum((s - 2) // 2, j, a)
-            tiles = sum(on_weights(s - 1, a) for a in range(RG))
-            if tiles == 2:
-                for j in range(2):
-                    weight_sum(s - 1, j, False)
-                    aggregate(s - 2, 2 * j, 2)
-                for j in range(2):
-                    weight_sum(s - 1, 2 + j, j == 1)
-                    project(project_at[s], ((4, 5, 0), (1, 2, 3))[j])
+                nc.vector.tensor_copy(
+                    out=nf_grp[:].rearrange("p (c d t) -> p c d t", c=2, t=4),
+                    in_=nf_raw[:].rearrange("p c (t d) -> p c d t", t=4),
+                )
+                sort(1, 0, 2)
+                nc.vector.quantize_mx(out=nf_codes[:].bitcast(FP8X4), scales=nf_scales[:], in_=nf_grp[:])
+            if s >= 3 and s % 2 == 1:
+                turn_supports((s - 3) // 2)
+            if s >= 4 and s % 2 == 0:
+                turn_sums((s - 4) // 2)
+                relation_part((s - 4) // 2)
+            if last:
+                turn_sums(HALVES - 2)
+                relation_part(HALVES - 2)
+            if 3 <= w < 15 and w % 4 in (3, 0):
+                turn_weights((w - 3) // 4 * 2 + (w - 3) % 4)
+            if 0 <= w < 12 and w % 2 == 0:
+                weight_values(w // 4, w // 2 % 2)
+            if 5 <= w < 17 and w % 4 == 1:
+                quantise_weights((w - 5) // 4)
+            if s >= 5 and s % 2 == 1:
+                quantise_nodes((s - 5) // 2)
+            if s >= 7 and s % 4 == 3:
+                quantise_relation((s - 7) // 4)
+            if last:
+                quantise(s, 0, 2)
+                quantise(s, 2, 2)
             else:
-                if tiles:
-                    weight_sum(s - 1, 0, False)
-                if s >= 2:
-                    aggregate(s - 2, 0, RG)
-                if tiles:
-                    weight_sum(s - 1, 1, True)
-                if s in project_at:
-                    project(project_at[s], (4, 5, 0, 1, 2, 3))
-            if s >= 2:
-                keep_supports(s - 2)
-            if tiles:
-                keep_sums(s - 1, tiles)
-            if s in project_at:
-                store(project_at[s])
-            if 3 <= s < STEPS - 1 and s % 2 == 1:
-                hh = (s - 3) // 2
-                collect_sums(hh)
-                relation_part(hh, sums[hh], nc.gpsimd)
-            if s + 1 < STEPS:
-                row_sum(s + 1, RG - 1)
-                if s % 2 == 0:
-                    spread_sums(s // 2)
-            if s < 2:
                 quantise(s)
-            if s + 2 < STEPS:
-                for a in range(RG - 1):
-                    if not unsorted(s + 2, a) and not on_scalar(s + 2, a):
-                        row_sum(s + 2, a)
+            if s == 0:
+                sort(1, 2, 2)
+            if s >= 1:
+                aggregate(s - 1)
+                keep_supports(s - 1)
+            if s in project_at:
+                project(project_at[s], all_passes)
+                store(project_at[s])
+            if s >= 1:
+                row_sums(s - 1)
+                keep_sums(s - 1)
 
         s, hh, it = STEPS - 1, HALVES - 1, IT - 1
-        aggregate(s - 1, 0, RG)
-        quantise(s, 0, 2)
-        collect_sums(hh - 1)
-        quantise(s, 2, 2)
-        quantise_nodes(it - 1)
-        keep_supports(s - 1)
-        turn_sums(hh)
-        aggregate(s, 0, RG)
+        row_sums(s)
+        keep_sums(s)
+        aggregate(s)
         keep_supports(s)
-        turn_supports(hh - 1)
+        quantise_nodes(hh - 1)
+        turn_sums(hh)
+        relation_part(hh)
+        project(it - 1, all_passes)
         turn_supports(hh)
-        project(it - 1, (4, 5, 0, 1, 2, 3))
         store(it - 1)
-        relation_part(hh - 1, sums[hh - 1], nc.vector)
-        relation_part(hh, sbank[hh], nc.vector)
         quantise_relation(it)
-        quantise_nodes(it, 0, 2)
-        project(it, (4, 5, 0, 1))
-        quantise_nodes(it, 2, 2)
-        project(it, (2, 3))
+        project(it, all_passes[:4])
+        quantise_nodes(hh)
+        project(it, all_passes[4:])
         store(it)

@@ -17,7 +17,7 @@ STEPS = IT * GROUPS
 HALVES = STEPS // 2
 SPREAD = DR // 4
 PREFETCH = 5
-W0 = 2
+W0 = 3
 FIRST_PROJECT = W0 + 14
 PROJECT_LAG = 8
 
@@ -28,6 +28,7 @@ U8 = mybir.dt.uint8
 FP8 = mybir.dt.float8_e4m3fn
 FP8X4 = mybir.dt.float8_e4m3fn_x4
 MULT = mybir.AluOpType.mult
+ADD = mybir.AluOpType.add
 
 FLOPS = 2 * (R * N * N * DE + N * R * F * NB)
 
@@ -47,7 +48,7 @@ def tile_relationalgraphconvolution_pa_kernel(
 
         ident = keep.tile([P, P], F32, name="ident", align_bytes=64)
         make_identity(nc, ident[:])
-        rep = [keep.tile([P, P], F32, name="rep%d" % h, align_bytes=64) for h in range(2)]
+        rep = [keep.tile([P, 2 * P], F32, name="rep%d" % h, align_bytes=64) for h in range(2)]
         ones = keep.tile([P, SPREAD], BF16, name="ones", align_bytes=64)
         nc.vector.memset(ones[:], 1.0)
         nf_raw = keep.tile([P, 2, 4 * DE], BF16, name="nf_raw", align_bytes=64)
@@ -69,6 +70,7 @@ def tile_relationalgraphconvolution_pa_kernel(
         scales = {}
         mx = {}
         sbank = {}
+        sums = {}
         supn = {}
         sgn = {}
         sgr = {}
@@ -191,22 +193,37 @@ def tile_relationalgraphconvolution_pa_kernel(
         def row_sums(s):
             wbank[s] = ring.tile([P, 512], F32, name="bank")
             for a in range(RG):
-                for j in range(8):
-                    c0 = a * N + j // 4 * 512
-                    nc.tensor.matmul(
-                        wbank[s][:, a * SPREAD : (a + 1) * SPREAD],
-                        lhsT=grp[s][:, c0 + j % 4 : c0 + 512 : 4],
-                        rhs=ones[:],
-                        start=(j == 0),
-                        stop=(j == 7),
-                    )
+                for v in range(2):
+                    k0 = (v * RG + a) * SPREAD
+                    for j in range(4):
+                        c0 = a * N + j // 2 * 512 + v * 256
+                        nc.tensor.matmul(
+                            wbank[s][:, k0 : k0 + SPREAD],
+                            lhsT=grp[s][:, c0 + j % 2 : c0 + 256 : 2],
+                            rhs=ones[:],
+                            start=(j == 0),
+                            stop=(j == 3),
+                        )
 
         def keep_sums(s):
-            nc.scalar.copy(out=rep[s // 2 % 2][:, s % 2 * 64 : s % 2 * 64 + 64], in_=wbank[s][:, 0:64])
+            nc.scalar.copy(
+                out=rep[s // 2 % 2][:].rearrange("p (v g m) -> p v g m", v=2, g=2)[:, :, s % 2, :],
+                in_=wbank[s][:, 0:P].rearrange("p (v m) -> p v m", v=2),
+            )
 
         def turn_sums(hh):
             sbank[hh] = ring.tile([P, 512], F32, name="bank")
-            nc.tensor.transpose(sbank[hh][:, 0:P], rep[hh % 2][:], ident[:])
+            for v in range(2):
+                nc.tensor.transpose(sbank[hh][:, v * P : (v + 1) * P], rep[hh % 2][:, v * P : (v + 1) * P], ident[:])
+
+        def collect_sums(hh):
+            sums[hh] = work.tile([P, P], F32, name="sums", align_bytes=64)
+            nc.vector.tensor_reduce(
+                out=sums[hh][:],
+                in_=sbank[hh][:, 0 : 2 * P].rearrange("p (i u) -> p i u", u=2),
+                axis=mybir.AxisListType.X,
+                op=ADD,
+            )
 
         def relation_part(hh):
             it, h = hh // 2, hh % 2
@@ -214,7 +231,7 @@ def tile_relationalgraphconvolution_pa_kernel(
                 sgr[it] = work.tile([P, 1024], BF16, name="sgr", align_bytes=64)
             nc.vector.tensor_tensor(
                 out=sgr[it][:, h * 512 : (h + 1) * 512].rearrange("p (i t) -> p i t", t=4),
-                in0=sbank[hh][:, 0:P].unsqueeze(2).to_broadcast([P, P, 4]),
+                in0=sums[hh][:].unsqueeze(2).to_broadcast([P, P, 4]),
                 in1=relf[:, h, :].unsqueeze(1).to_broadcast([P, P, 4]),
                 op=MULT,
             )
@@ -304,6 +321,8 @@ def tile_relationalgraphconvolution_pa_kernel(
                 load(s + PREFETCH)
             if s in (0, 3):
                 load_weights(1 + s // 3)
+            if s >= 4 and s % 2 == 0:
+                relation_part((s - 4) // 2)
             if 1 <= s < STEPS - 1:
                 sort(s + 1)
             for a in range(RG):
@@ -312,7 +331,7 @@ def tile_relationalgraphconvolution_pa_kernel(
                 if last:
                     to_vector = a % 2 == 1
                 else:
-                    to_vector = a == 3 and s % 4 != 2 and not (0 <= w < 12 and w % 2 == 0)
+                    to_vector = a == 3 and s % 4 == 0
                 empty(s, a, turn(s, a), nc.vector.tensor_copy if to_vector else nc.scalar.copy)
             if s == 0:
                 nc.vector.tensor_copy(
@@ -322,13 +341,12 @@ def tile_relationalgraphconvolution_pa_kernel(
                 sort(1, 0, 2)
                 nc.vector.quantize_mx(out=nf_codes[:].bitcast(FP8X4), scales=nf_scales[:], in_=nf_grp[:])
             if s >= 3 and s % 2 == 1:
-                turn_supports((s - 3) // 2)
+                turn_sums((s - 3) // 2)
+                collect_sums((s - 3) // 2)
             if s >= 4 and s % 2 == 0:
-                turn_sums((s - 4) // 2)
-                relation_part((s - 4) // 2)
+                turn_supports((s - 4) // 2)
             if last:
-                turn_sums(HALVES - 2)
-                relation_part(HALVES - 2)
+                turn_supports(HALVES - 2)
             if 3 <= w < 15 and w % 4 in (3, 0):
                 turn_weights((w - 3) // 4 * 2 + (w - 3) % 4)
             if 0 <= w < 12 and w % 2 == 0:
@@ -361,8 +379,10 @@ def tile_relationalgraphconvolution_pa_kernel(
         keep_sums(s)
         aggregate(s)
         keep_supports(s)
-        quantise_nodes(hh - 1)
+        relation_part(hh - 1)
         turn_sums(hh)
+        collect_sums(hh)
+        quantise_nodes(hh - 1)
         relation_part(hh)
         project(it - 1, all_passes)
         turn_supports(hh)

@@ -17,7 +17,7 @@ STEPS = IT * GROUPS
 HALVES = STEPS // 2
 SPREAD = DR // 4
 PREFETCH = 5
-W0 = 3
+W0 = 5
 FIRST_PROJECT = W0 + 14
 PROJECT_LAG = 8
 
@@ -33,6 +33,10 @@ ADD = mybir.AluOpType.add
 FLOPS = 2 * (R * N * N * DE + N * R * F * NB)
 
 
+def summed_on_vector(s):
+    return RG if s == STEPS - 1 else 0 if s < 3 else 2 * (s % 2) if s <= FIRST_PROJECT else 2
+
+
 def tile_relationalgraphconvolution_pa_kernel(
     tc, node_features, relation_features, adj, Wb_bytes, Wb_scale, out
 ):
@@ -42,13 +46,22 @@ def tile_relationalgraphconvolution_pa_kernel(
         rawp = ctx.enter_context(tc.tile_pool(name="rawp", bufs=PREFETCH + 1))
         work = ctx.enter_context(tc.tile_pool(name="work", bufs=2))
         three = ctx.enter_context(tc.tile_pool(name="three", bufs=3))
+        onep = ctx.enter_context(tc.tile_pool(name="onep", bufs=6))
         four = ctx.enter_context(tc.tile_pool(name="four", bufs=4))
-        ring = ctx.enter_context(tc.psum_pool(name="ring", bufs=8))
+        ring = ctx.enter_context(tc.psum_pool(name="ring", bufs=7))
+        sump = ctx.enter_context(tc.psum_pool(name="sump", bufs=1))
         ctx.enter_context(tc.manual_schedule())
 
         ident = keep.tile([P, P], F32, name="ident", align_bytes=64)
         make_identity(nc, ident[:])
-        rep = [keep.tile([P, 2 * P], F32, name="rep%d" % h, align_bytes=64) for h in range(2)]
+        rs = keep.tile([P, STEPS * RG], F32, name="rs", align_bytes=64)
+        rep = {}
+        for hh in range(HALVES):
+            key = (hh % 2, summed_on_vector(2 * hh), summed_on_vector(2 * hh + 1))
+            if key not in rep:
+                rep[key] = keep.tile([P, 3 * P], F32, name="rep%d%d%d" % key, align_bytes=64)
+                if key[1] + key[2] > 0:
+                    nc.vector.memset(rep[key][:], 0.0)
         ones = keep.tile([P, SPREAD], BF16, name="ones", align_bytes=64)
         nc.vector.memset(ones[:], 1.0)
         nf_raw = keep.tile([P, 2, 4 * DE], BF16, name="nf_raw", align_bytes=64)
@@ -111,16 +124,41 @@ def tile_relationalgraphconvolution_pa_kernel(
                 in_=sc[r0 : r0 + n, f0 : f0 + width].partition_broadcast(P),
             )
 
-        def sort(s, a0=0, n=RG):
-            if n == RG:
+        def sort(s, a0, n):
+            if n > 1:
                 dst = three.tile([P, n * N], BF16, name="perm", align_bytes=64)
             else:
-                dst = four.tile([P, n * N], BF16, name="permpart", align_bytes=64)
+                dst = onep.tile([P, N], BF16, name="permone", align_bytes=64)
             for a in range(n):
                 perm[s, a0 + a] = (dst, n, a)
             nc.vector.tensor_copy(
                 out=dst[:].rearrange("p (u q f) -> p u q f", u=2, f=16),
                 in_=raw[s][:, a0 * N : (a0 + n) * N].rearrange("p (q u f) -> p u q f", u=2, f=16),
+            )
+
+        def sort_and_sum(s, a):
+            dst = onep.tile([P, N], BF16, name="permone", align_bytes=64)
+            perm[s, a] = (dst, 1, 0)
+            nc.vector.tensor_scalar(
+                out=dst[:].rearrange("p (u q f) -> p u q f", u=2, f=16),
+                in0=raw[s][:, a * N : (a + 1) * N].rearrange("p (q u f) -> p u q f", u=2, f=16),
+                scalar1=1.0,
+                scalar2=None,
+                op0=MULT,
+                op1=ADD,
+                accum_out=rs[:, s * RG + a : s * RG + a + 1],
+            )
+
+        def spread(hh):
+            return rep[hh % 2, summed_on_vector(2 * hh), summed_on_vector(2 * hh + 1)]
+
+        def spread_sums(s0, steps):
+            n = summed_on_vector(s0)
+            g0 = s0 % 2
+            dst = spread(s0 // 2)[:, 2 * P : 3 * P].rearrange("p (g a q) -> p g a q", g=2, q=SPREAD)
+            src = rs[:].rearrange("p (s a) -> p s a", a=RG)[:, s0 : s0 + steps, 0:n]
+            nc.scalar.copy(
+                out=dst[:, g0 : g0 + steps, 0:n, :], in_=src.unsqueeze(3).to_broadcast([P, steps, n, SPREAD])
             )
 
         def turn(s, a):
@@ -152,9 +190,10 @@ def tile_relationalgraphconvolution_pa_kernel(
                 in_=grp[s][:, a0 * N : (a0 + n) * N],
             )
 
-        def aggregate(s):
-            mx[s] = ring.tile([P, 512], F32, name="bank")
-            for a in range(RG):
+        def aggregate(s, a0=0, n=RG):
+            if a0 == 0:
+                mx[s] = ring.tile([P, 512], F32, name="bank")
+            for a in range(a0, a0 + n):
                 for c in range(2):
                     cols = slice(a * 256 + c * P, a * 256 + (c + 1) * P)
                     nc.tensor.matmul_mx(
@@ -176,23 +215,22 @@ def tile_relationalgraphconvolution_pa_kernel(
                 in_=mx[s][:].rearrange("p (q u e) -> p u q e", u=2, e=2),
             )
 
-        def turn_supports(hh):
-            it, q0 = hh // 2, 2 * (hh % 2)
+        def turn_supports(hh, g0=0, n=2):
+            it, q0 = hh // 2, 2 * (hh % 2) + g0
             if q0 == 0:
                 sgn[it] = work.tile([P, 2048], BF16, name="sgn", align_bytes=64)
             bank = ring.tile([P, 512], F32, name="bank")
-            for b in range(2):
-                for u in range(2):
-                    k0 = (b * 2 + u) * P
-                    nc.tensor.transpose(bank[:, k0 : k0 + P], supn[hh][:].bitcast(F32)[:, k0 : k0 + P], ident[:])
+            for k in range(2 * n):
+                w0 = (2 * g0 + k) * P
+                nc.tensor.transpose(bank[:, k * P : (k + 1) * P], supn[hh][:].bitcast(F32)[:, w0 : w0 + P], ident[:])
             nc.scalar.copy(
-                out=sgn[it][:, q0 * 512 : (q0 + 2) * 512].bitcast(F32).rearrange("p (b i u) -> p b i u", b=2, u=2),
-                in_=bank[:].rearrange("p (b u i) -> p b i u", b=2, u=2),
+                out=sgn[it][:, q0 * 512 : (q0 + n) * 512].bitcast(F32).rearrange("p (b i u) -> p b i u", b=n, u=2),
+                in_=bank[:, 0 : n * 256].rearrange("p (b u i) -> p b i u", b=n, u=2),
             )
 
         def row_sums(s):
             wbank[s] = ring.tile([P, 512], F32, name="bank")
-            for a in range(RG):
+            for a in range(summed_on_vector(s), RG):
                 for v in range(2):
                     k0 = (v * RG + a) * SPREAD
                     for j in range(4):
@@ -206,15 +244,25 @@ def tile_relationalgraphconvolution_pa_kernel(
                         )
 
         def keep_sums(s):
+            m0 = summed_on_vector(s) * SPREAD
             nc.scalar.copy(
-                out=rep[s // 2 % 2][:].rearrange("p (v g m) -> p v g m", v=2, g=2)[:, :, s % 2, :],
-                in_=wbank[s][:, 0:P].rearrange("p (v m) -> p v m", v=2),
+                out=spread(s // 2)[:, 0 : 2 * P].rearrange("p (v g m) -> p v g m", v=2, g=2)[:, :, s % 2, m0:],
+                in_=wbank[s][:, 0:P].rearrange("p (v m) -> p v m", v=2)[:, :, m0:],
             )
 
         def turn_sums(hh):
-            sbank[hh] = ring.tile([P, 512], F32, name="bank")
-            for v in range(2):
-                nc.tensor.transpose(sbank[hh][:, v * P : (v + 1) * P], rep[hh % 2][:, v * P : (v + 1) * P], ident[:])
+            pool = sump if hh < HALVES - 1 else ring
+            sbank[hh] = pool.tile([P, 512], F32, name="bank")
+            parts = 3 if summed_on_vector(2 * hh) + summed_on_vector(2 * hh + 1) else 2
+            for v in range(parts):
+                nc.tensor.matmul(
+                    sbank[hh][:, v * P : (v + 1) * P] if v < 2 else sbank[hh][:, 0 : 2 * P : 2],
+                    lhsT=spread(hh)[:, v * P : (v + 1) * P],
+                    rhs=ident[:],
+                    start=(v == 0),
+                    stop=(v == parts - 1),
+                    is_transpose=True,
+                )
 
         def collect_sums(hh):
             sums[hh] = work.tile([P, P], F32, name="sums", align_bytes=64)
@@ -225,11 +273,11 @@ def tile_relationalgraphconvolution_pa_kernel(
                 op=ADD,
             )
 
-        def relation_part(hh):
+        def relation_part(hh, engine):
             it, h = hh // 2, hh % 2
             if h == 0:
                 sgr[it] = work.tile([P, 1024], BF16, name="sgr", align_bytes=64)
-            nc.vector.tensor_tensor(
+            engine.tensor_tensor(
                 out=sgr[it][:, h * 512 : (h + 1) * 512].rearrange("p (i t) -> p i t", t=4),
                 in0=sums[hh][:].unsqueeze(2).to_broadcast([P, P, 4]),
                 in1=relf[:, h, :].unsqueeze(1).to_broadcast([P, P, 4]),
@@ -241,16 +289,16 @@ def tile_relationalgraphconvolution_pa_kernel(
                 out=scodes[it][:, 4 * P : 6 * P].bitcast(FP8X4), scales=sscales[it][:, 4 * P : 6 * P], in_=sgr[it][:]
             )
 
-        def quantise_nodes(hh):
-            it, q0 = hh // 2, 2 * (hh % 2)
+        def quantise_nodes(hh, g0=0, n=2):
+            it, q0 = hh // 2, 2 * (hh % 2) + g0
             if q0 == 0:
                 scodes[it] = four.tile([P, 6 * P], U32, name="scodes", align_bytes=64)
                 sscales[it] = four.tile([P, 6 * P], U8, name="sscales", align_bytes=64)
-            cols = slice(q0 * P, (q0 + 2) * P)
+            cols = slice(q0 * P, (q0 + n) * P)
             nc.vector.quantize_mx(
                 out=scodes[it][:, cols].bitcast(FP8X4),
                 scales=sscales[it][:, cols],
-                in_=sgn[it][:, q0 * 512 : (q0 + 2) * 512],
+                in_=sgn[it][:, q0 * 512 : (q0 + n) * 512],
             )
 
         def project(it, passes):
@@ -304,49 +352,55 @@ def tile_relationalgraphconvolution_pa_kernel(
 
         all_passes = (0, 1, 4, 5, 2, 3)
         load(0, 4)
-        load_features()
         load(1, 2)
-        nc.sync.dma_start(out=relf[:], in_=relation_features[0].rearrange("(h r) (q t) -> (r q) h t", h=2, t=4))
-        load(2)
-        load_weights(0)
+        load_features()
+        load(2, 2)
         for s in range(3, PREFETCH):
             load(s)
+        nc.sync.dma_start(out=relf[:], in_=relation_features[0].rearrange("(h r) (q t) -> (r q) h t", h=2, t=4))
 
-        project_at = {max(4 * it + PROJECT_LAG, it + FIRST_PROJECT): it for it in range(IT)}
+        project_at = {max(4 * it + PROJECT_LAG, 2 * it + FIRST_PROJECT): it for it in range(IT)}
 
-        for s in range(STEPS):
+        def sort_step(s):
+            n = summed_on_vector(s)
+            for a in range(n):
+                sort_and_sum(s, a)
+            if s < 3:
+                for a in range(n, RG):
+                    sort(s, a, 1)
+            elif n < RG:
+                sort(s, n, RG - n)
+
+        def spread_half(hh):
+            n0, n1 = summed_on_vector(2 * hh), summed_on_vector(2 * hh + 1)
+            if n0 == n1:
+                spread_sums(2 * hh, 2)
+            else:
+                for s in (2 * hh, 2 * hh + 1):
+                    if summed_on_vector(s):
+                        spread_sums(s, 1)
+
+        sort_step(0)
+        for s in range(STEPS - 1):
             w = s - W0
-            last = s == STEPS - 1
+            if w + 4 in (0, 3, 6):
+                load_weights((w + 4) // 3)
             if s + PREFETCH < STEPS:
                 load(s + PREFETCH)
-            if s in (0, 3):
-                load_weights(1 + s // 3)
-            if s >= 4 and s % 2 == 0:
-                relation_part((s - 4) // 2)
-            if 1 <= s < STEPS - 1:
-                sort(s + 1)
+            sort_step(s + 1)
             for a in range(RG):
-                if s == 0:
-                    sort(0, a, 1)
-                if last:
-                    to_vector = a % 2 == 1
-                else:
-                    to_vector = a == 3 and s % 4 == 0
-                empty(s, a, turn(s, a), nc.vector.tensor_copy if to_vector else nc.scalar.copy)
+                empty(s, a, turn(s, a))
             if s == 0:
                 nc.vector.tensor_copy(
                     out=nf_grp[:].rearrange("p (c d t) -> p c d t", c=2, t=4),
                     in_=nf_raw[:].rearrange("p c (t d) -> p c d t", t=4),
                 )
-                sort(1, 0, 2)
+                quantise(0)
                 nc.vector.quantize_mx(out=nf_codes[:].bitcast(FP8X4), scales=nf_scales[:], in_=nf_grp[:])
             if s >= 3 and s % 2 == 1:
                 turn_sums((s - 3) // 2)
-                collect_sums((s - 3) // 2)
             if s >= 4 and s % 2 == 0:
                 turn_supports((s - 4) // 2)
-            if last:
-                turn_supports(HALVES - 2)
             if 3 <= w < 15 and w % 4 in (3, 0):
                 turn_weights((w - 3) // 4 * 2 + (w - 3) % 4)
             if 0 <= w < 12 and w % 2 == 0:
@@ -357,33 +411,48 @@ def tile_relationalgraphconvolution_pa_kernel(
                 quantise_nodes((s - 5) // 2)
             if s >= 7 and s % 4 == 3:
                 quantise_relation((s - 7) // 4)
-            if last:
-                quantise(s, 0, 2)
-                quantise(s, 2, 2)
-            else:
+            if s >= 1:
                 quantise(s)
-            if s == 0:
-                sort(1, 2, 2)
+            if s >= 3 and s % 2 == 1:
+                collect_sums((s - 3) // 2)
+                relation_part((s - 3) // 2, nc.gpsimd)
+            if s == 1:
+                row_sums(0)
+                keep_sums(0)
             if s >= 1:
                 aggregate(s - 1)
                 keep_supports(s - 1)
             if s in project_at:
                 project(project_at[s], all_passes)
                 store(project_at[s])
-            if s >= 1:
+            if s >= 2:
                 row_sums(s - 1)
                 keep_sums(s - 1)
+            if s % 2 == 1 and s > 1:
+                spread_half(s // 2)
 
         s, hh, it = STEPS - 1, HALVES - 1, IT - 1
-        row_sums(s)
-        keep_sums(s)
+        row_sums(s - 1)
+        keep_sums(s - 1)
+        spread_half(hh)
+        quantise_nodes(hh - 2)
+        quantise_relation(it - 1)
+        for a in range(RG):
+            empty(s, a, turn(s, a), nc.vector.tensor_copy if a % 2 else nc.scalar.copy)
+        quantise(s, 0, 2)
+        quantise(s, 2, 2)
+        turn_sums(hh - 1)
+        collect_sums(hh - 1)
+        turn_supports(hh - 1)
+        turn_sums(hh)
+        aggregate(s - 1)
+        keep_supports(s - 1)
         aggregate(s)
         keep_supports(s)
-        relation_part(hh - 1)
-        turn_sums(hh)
         collect_sums(hh)
+        relation_part(hh - 1, nc.vector)
         quantise_nodes(hh - 1)
-        relation_part(hh)
+        relation_part(hh, nc.vector)
         project(it - 1, all_passes)
         turn_supports(hh)
         store(it - 1)

@@ -14,12 +14,12 @@ IT = N // P
 RG = 4
 GROUPS = R // RG
 STEPS = IT * GROUPS
-HALVES = STEPS // 2
-SPREAD = DR // 4
+GROUP = 8
+PASSES = F // 32
 PREFETCH = 5
-W0 = 5
-FIRST_PROJECT = W0 + 14
-PROJECT_LAG = 8
+W0 = 3
+FIRST_PROJECT = W0 + 13
+PROJECT_LAG = 10
 
 F32 = mybir.dt.float32
 BF16 = mybir.dt.bfloat16
@@ -29,12 +29,13 @@ FP8 = mybir.dt.float8_e4m3fn
 FP8X4 = mybir.dt.float8_e4m3fn_x4
 MULT = mybir.AluOpType.mult
 ADD = mybir.AluOpType.add
+AXIS_X = mybir.AxisListType.X
 
 FLOPS = 2 * (R * N * N * DE + N * R * F * NB)
 
 
 def summed_on_vector(s):
-    return RG if s == STEPS - 1 else 0 if s < 3 else 2 * (s % 2) if s <= FIRST_PROJECT else 2
+    return RG if s == STEPS - 1 else int(s >= FIRST_PROJECT)
 
 
 def tile_relationalgraphconvolution_pa_kernel(
@@ -44,37 +45,45 @@ def tile_relationalgraphconvolution_pa_kernel(
     with ExitStack() as ctx:
         keep = ctx.enter_context(tc.tile_pool(name="keep", bufs=1))
         rawp = ctx.enter_context(tc.tile_pool(name="rawp", bufs=PREFETCH + 1))
-        work = ctx.enter_context(tc.tile_pool(name="work", bufs=2))
+        onep = ctx.enter_context(tc.tile_pool(name="onep", bufs=8))
+        two = ctx.enter_context(tc.tile_pool(name="two", bufs=2))
         three = ctx.enter_context(tc.tile_pool(name="three", bufs=3))
-        onep = ctx.enter_context(tc.tile_pool(name="onep", bufs=6))
         four = ctx.enter_context(tc.tile_pool(name="four", bufs=4))
-        ring = ctx.enter_context(tc.psum_pool(name="ring", bufs=7))
+        ring = ctx.enter_context(tc.psum_pool(name="ring", bufs=6))
         sump = ctx.enter_context(tc.psum_pool(name="sump", bufs=1))
         ctx.enter_context(tc.manual_schedule())
 
         ident = keep.tile([P, P], F32, name="ident", align_bytes=64)
         make_identity(nc, ident[:])
         rs = keep.tile([P, STEPS * RG], F32, name="rs", align_bytes=64)
+        patterns = [tuple(summed_on_vector(GROUPS * it + g) for g in range(GROUPS)) for it in range(IT)]
         rep = {}
-        for hh in range(HALVES):
-            key = (hh % 2, summed_on_vector(2 * hh), summed_on_vector(2 * hh + 1))
+        for key in patterns:
             if key not in rep:
-                rep[key] = keep.tile([P, 3 * P], F32, name="rep%d%d%d" % key, align_bytes=64)
-                if key[1] + key[2] > 0:
+                rep[key] = keep.tile([P, 3 * P], F32, name="rep%d%d%d%d" % key, align_bytes=64)
+                if sum(key):
                     nc.vector.memset(rep[key][:], 0.0)
-        ones = keep.tile([P, SPREAD], BF16, name="ones", align_bytes=64)
+        ones = keep.tile([P, GROUP], BF16, name="ones", align_bytes=64)
         nc.vector.memset(ones[:], 1.0)
+        one = keep.tile([P, 1], F32, name="one", align_bytes=64)
+        nc.vector.memset(one[:], 1.0)
+        pick = keep.tile([P, GROUP], F32, name="pick", align_bytes=64)
+        nc.vector.tensor_reduce(
+            out=pick[:], in_=ident[:].rearrange("p (g x) -> p x g", x=GROUP), axis=AXIS_X, op=ADD
+        )
         nf_raw = keep.tile([P, 2, 4 * DE], BF16, name="nf_raw", align_bytes=64)
         nf_grp = keep.tile([P, 2 * 4 * DE], BF16, name="nf_grp", align_bytes=64)
         nf_codes = keep.tile([P, 2 * DE], U32, name="nf_codes", align_bytes=64)
         nf_scales = keep.tile([P, 2 * DE], U8, name="nf_scales", align_bytes=64)
-        relf = keep.tile([P, 2, 4], BF16, name="relf", align_bytes=64)
-        w_bytes = keep.tile([P, 2 * R * F], U8, name="w_bytes", align_bytes=64)
-        w_scale = keep.tile([P, R * F], F32, name="w_scale", align_bytes=64)
-        w_val = keep.tile([P, 2 * R * F], BF16, name="w_val", align_bytes=64)
-        w_grp = keep.tile([P, 6 * NB * 4], BF16, name="w_grp", align_bytes=64)
-        w_codes = keep.tile([P, 6 * NB], U32, name="w_codes", align_bytes=64)
-        w_scales = keep.tile([P, 6 * NB], U8, name="w_scales", align_bytes=64)
+        rel_rows = keep.tile([P, DR], BF16, name="rel_rows", align_bytes=64)
+        relf = keep.tile([P, 2 * 4], F32, name="relf", align_bytes=64)
+        scale_rows = keep.tile([P, F], F32, name="scale_rows", align_bytes=64)
+        w_scale = keep.tile([P, PASSES * 4], F32, name="w_scale", align_bytes=64)
+        w_bytes = [keep.tile([P, R * F], U8, name="w_bytes%d" % h, align_bytes=64) for h in range(2)]
+        w_val = [keep.tile([P, R * F], BF16, name="w_val%d" % h, align_bytes=64) for h in range(2)]
+        w_grp = keep.tile([P, PASSES * NB * 4], BF16, name="w_grp", align_bytes=64)
+        w_codes = keep.tile([P, PASSES * NB], U32, name="w_codes", align_bytes=64)
+        w_scales = keep.tile([P, PASSES * NB], U8, name="w_scales", align_bytes=64)
 
         raw = {}
         perm = {}
@@ -82,6 +91,7 @@ def tile_relationalgraphconvolution_pa_kernel(
         codes = {}
         scales = {}
         mx = {}
+        wbank = {}
         sbank = {}
         sums = {}
         supn = {}
@@ -90,7 +100,7 @@ def tile_relationalgraphconvolution_pa_kernel(
         scodes = {}
         sscales = {}
         obank = {}
-        wbank = {}
+        tbank = {}
 
         def load(s, pieces=1):
             it, g = s // GROUPS, s % GROUPS
@@ -109,24 +119,27 @@ def tile_relationalgraphconvolution_pa_kernel(
                 for u in range(2):
                     nc.sync.dma_start(out=nf_raw[:, c, u * 2 * DE : (u + 1) * 2 * DE], in_=runs[c, u])
 
-        def load_weights(pair):
-            r0, n, f0, width = (0, R, DE, DR) if pair == 2 else (pair * 8, 8, 0, DE)
-            for h in range(2):
-                c0 = h * R * F + pair * 1024
-                rows = Wb_bytes[h * P : (h + 1) * P, :].rearrange("n (r f) -> n r f", f=F)
-                nc.sync.dma_start(
-                    out=w_bytes[:, c0 : c0 + 1024].rearrange("p (r d) -> p r d", d=width),
-                    in_=rows[:, r0 : r0 + n, f0 : f0 + width],
-                )
-            sc = Wb_scale.rearrange("o (r f) -> (o r) f", f=F)
-            nc.sync.dma_start(
-                out=w_scale[:, pair * 1024 : (pair + 1) * 1024].rearrange("p (r d) -> p r d", d=width),
-                in_=sc[r0 : r0 + n, f0 : f0 + width].partition_broadcast(P),
+        def load_rows(dst, rows):
+            nc.sync.dma_start(out=dst[:], in_=rows.partition_broadcast(GROUP).rearrange("x r f -> r x f"))
+
+        def pick_own(dst, rows, width):
+            masked = two.tile([P, width], F32, name="masked", align_bytes=64)
+            nc.vector.tensor_tensor(
+                out=masked[:].rearrange("p (m x e) -> p m x e", x=GROUP, e=2),
+                in0=rows[:].rearrange("p (m x e) -> p m x e", x=GROUP, e=2),
+                in1=pick[:].unsqueeze(1).unsqueeze(3).to_broadcast([P, width // 16, GROUP, 2]),
+                op=MULT,
+            )
+            return lambda: nc.vector.tensor_reduce(
+                out=dst[:].rearrange("p (m e) -> p m e", e=2),
+                in_=masked[:].rearrange("p (m x e) -> p m e x", x=GROUP, e=2),
+                axis=AXIS_X,
+                op=ADD,
             )
 
         def sort(s, a0, n):
             if n > 1:
-                dst = three.tile([P, n * N], BF16, name="perm", align_bytes=64)
+                dst = four.tile([P, n * N], BF16, name="perm", align_bytes=64)
             else:
                 dst = onep.tile([P, N], BF16, name="permone", align_bytes=64)
             for a in range(n):
@@ -139,27 +152,22 @@ def tile_relationalgraphconvolution_pa_kernel(
         def sort_and_sum(s, a):
             dst = onep.tile([P, N], BF16, name="permone", align_bytes=64)
             perm[s, a] = (dst, 1, 0)
+            sorted_words = dst[:].rearrange("p (u q f) -> p u q f", u=2, f=16)
+            row = raw[s][:, a * N : (a + 1) * N].rearrange("p (q u f) -> p u q f", u=2, f=16)
+            total = rs[:, s * RG + a : s * RG + a + 1]
             nc.vector.tensor_scalar(
-                out=dst[:].rearrange("p (u q f) -> p u q f", u=2, f=16),
-                in0=raw[s][:, a * N : (a + 1) * N].rearrange("p (q u f) -> p u q f", u=2, f=16),
-                scalar1=1.0,
-                scalar2=None,
-                op0=MULT,
-                op1=ADD,
-                accum_out=rs[:, s * RG + a : s * RG + a + 1],
+                out=sorted_words, in0=row, scalar1=1.0, scalar2=None, op0=MULT, op1=ADD, accum_out=total
             )
 
-        def spread(hh):
-            return rep[hh % 2, summed_on_vector(2 * hh), summed_on_vector(2 * hh + 1)]
-
-        def spread_sums(s0, steps):
-            n = summed_on_vector(s0)
-            g0 = s0 % 2
-            dst = spread(s0 // 2)[:, 2 * P : 3 * P].rearrange("p (g a q) -> p g a q", g=2, q=SPREAD)
-            src = rs[:].rearrange("p (s a) -> p s a", a=RG)[:, s0 : s0 + steps, 0:n]
-            nc.scalar.copy(
-                out=dst[:, g0 : g0 + steps, 0:n, :], in_=src.unsqueeze(3).to_broadcast([P, steps, n, SPREAD])
-            )
+        def sort_step(s):
+            n = summed_on_vector(s)
+            for a in range(summed_on_vector(s)):
+                sort_and_sum(s, a)
+            if s < 3:
+                for a in range(n, RG):
+                    sort(s, a, 1)
+            elif n < RG:
+                sort(s, n, RG - n)
 
         def turn(s, a):
             if a == 0:
@@ -191,13 +199,12 @@ def tile_relationalgraphconvolution_pa_kernel(
             )
 
         def aggregate(s, a0=0, n=RG):
-            if a0 == 0:
-                mx[s] = ring.tile([P, 512], F32, name="bank")
+            mx[s, a0] = ring.tile([P, 512], F32, name="bank")
             for a in range(a0, a0 + n):
                 for c in range(2):
                     cols = slice(a * 256 + c * P, a * 256 + (c + 1) * P)
                     nc.tensor.matmul_mx(
-                        out=mx[s][:, a * DE : (a + 1) * DE],
+                        out=mx[s, a0][:, (a - a0) * DE : (a - a0 + 1) * DE],
                         lhsT=codes[s][:, cols].bitcast(FP8X4),
                         lhsT_scale=scales[s][:, cols],
                         rhs=nf_codes[:, c * DE : (c + 1) * DE].bitcast(FP8X4),
@@ -206,104 +213,109 @@ def tile_relationalgraphconvolution_pa_kernel(
                         stop=(c == 1),
                     )
 
-        def keep_supports(s):
-            hh, g = s // 2, s % 2
-            if g == 0:
-                supn[hh] = three.tile([P, 1024], BF16, name="supn", align_bytes=64)
+        def keep_supports(s, a0=0, n=RG):
+            it, r0 = s // GROUPS, s % GROUPS * RG + a0
+            if r0 == 0:
+                supn[it] = two.tile([P, R * DE], BF16, name="supn", align_bytes=64)
             nc.scalar.copy(
-                out=supn[hh][:, g * 512 : (g + 1) * 512].rearrange("p (u q e) -> p u q e", u=2, e=2),
-                in_=mx[s][:].rearrange("p (q u e) -> p u q e", u=2, e=2),
+                out=supn[it][:].rearrange("p (m r f) -> p m r f", r=R, f=16)[:, :, r0 : r0 + n, :],
+                in_=mx[s, a0][:, 0 : n * DE].rearrange("p (a m f) -> p m a f", a=n, f=16),
             )
 
-        def turn_supports(hh, g0=0, n=2):
-            it, q0 = hh // 2, 2 * (hh % 2) + g0
-            if q0 == 0:
-                sgn[it] = work.tile([P, 2048], BF16, name="sgn", align_bytes=64)
+        def turn_supports(it, j, copy=nc.scalar.copy):
+            if j == 0:
+                sgn[it] = two.tile([P, 2048], BF16, name="sgn", align_bytes=64)
             bank = ring.tile([P, 512], F32, name="bank")
-            for k in range(2 * n):
-                w0 = (2 * g0 + k) * P
-                nc.tensor.transpose(bank[:, k * P : (k + 1) * P], supn[hh][:].bitcast(F32)[:, w0 : w0 + P], ident[:])
-            nc.scalar.copy(
-                out=sgn[it][:, q0 * 512 : (q0 + n) * 512].bitcast(F32).rearrange("p (b i u) -> p b i u", b=n, u=2),
-                in_=bank[:, 0 : n * 256].rearrange("p (b u i) -> p b i u", b=n, u=2),
+            for k in range(4):
+                w0 = (4 * j + k) * P
+                nc.tensor.transpose(bank[:, k * P : (k + 1) * P], supn[it][:].bitcast(F32)[:, w0 : w0 + P], ident[:])
+            copy(
+                out=sgn[it][:, j * 1024 : (j + 1) * 1024].bitcast(F32).rearrange("p (b i u) -> p b i u", b=2, u=2),
+                in_=bank[:].rearrange("p (b u i) -> p b i u", b=2, u=2),
             )
 
         def row_sums(s):
-            wbank[s] = ring.tile([P, 512], F32, name="bank")
+            it, g = s // GROUPS, s % GROUPS
+            if g == 0:
+                wbank[it] = sump.tile([P, 512], F32, name="wbank")
             for a in range(summed_on_vector(s), RG):
                 for v in range(2):
-                    k0 = (v * RG + a) * SPREAD
+                    k0 = v * P + (g * RG + a) * GROUP
                     for j in range(4):
                         c0 = a * N + j // 2 * 512 + v * 256
                         nc.tensor.matmul(
-                            wbank[s][:, k0 : k0 + SPREAD],
+                            wbank[it][:, k0 : k0 + GROUP],
                             lhsT=grp[s][:, c0 + j % 2 : c0 + 256 : 2],
                             rhs=ones[:],
                             start=(j == 0),
                             stop=(j == 3),
                         )
 
-        def keep_sums(s):
-            m0 = summed_on_vector(s) * SPREAD
-            nc.scalar.copy(
-                out=spread(s // 2)[:, 0 : 2 * P].rearrange("p (v g m) -> p v g m", v=2, g=2)[:, :, s % 2, m0:],
-                in_=wbank[s][:, 0:P].rearrange("p (v m) -> p v m", v=2)[:, :, m0:],
-            )
+        def runs_of(it):
+            key = patterns[it]
+            starts = [g for g in range(GROUPS) if g == 0 or key[g] != key[g - 1]]
+            return [(g0, g1, key[g0]) for g0, g1 in zip(starts, starts[1:] + [GROUPS])]
 
-        def turn_sums(hh):
-            pool = sump if hh < HALVES - 1 else ring
-            sbank[hh] = pool.tile([P, 512], F32, name="bank")
-            parts = 3 if summed_on_vector(2 * hh) + summed_on_vector(2 * hh + 1) else 2
+        def keep_sums(it):
+            dst = rep[patterns[it]][:, 0 : 2 * P].rearrange("p (v g m) -> p v g m", v=2, g=GROUPS)
+            src = wbank[it][:, 0 : 2 * P].rearrange("p (v g m) -> p v g m", v=2, g=GROUPS)
+            for g0, g1, n in runs_of(it):
+                if n < RG:
+                    nc.scalar.copy(out=dst[:, :, g0:g1, n * GROUP :], in_=src[:, :, g0:g1, n * GROUP :])
+
+        def spread_sums(it):
+            dst = rep[patterns[it]][:, 2 * P : 3 * P].rearrange("p (g a x) -> p g a x", g=GROUPS, x=GROUP)
+            src = rs[:, it * R : (it + 1) * R].rearrange("p (g a) -> p g a", a=RG)
+            for g0, g1, n in runs_of(it):
+                if n:
+                    nc.scalar.copy(
+                        out=dst[:, g0:g1, 0:n, :],
+                        in_=src[:, g0:g1, 0:n].unsqueeze(3).to_broadcast([P, g1 - g0, n, GROUP]),
+                    )
+
+        def turn_sums(it):
+            sbank[it] = sump.tile([P, 512], F32, name="sbank")
+            parts = 3 if sum(patterns[it]) else 2
             for v in range(parts):
                 nc.tensor.matmul(
-                    sbank[hh][:, v * P : (v + 1) * P] if v < 2 else sbank[hh][:, 0 : 2 * P : 2],
-                    lhsT=spread(hh)[:, v * P : (v + 1) * P],
+                    sbank[it][:, v * P : (v + 1) * P] if v < 2 else sbank[it][:, 0 : 2 * P : 2],
+                    lhsT=rep[patterns[it]][:, v * P : (v + 1) * P],
                     rhs=ident[:],
                     start=(v == 0),
                     stop=(v == parts - 1),
                     is_transpose=True,
                 )
 
-        def collect_sums(hh):
-            sums[hh] = work.tile([P, P], F32, name="sums", align_bytes=64)
+        def collect_sums(it):
+            sums[it] = two.tile([P, P], F32, name="sums", align_bytes=64)
             nc.vector.tensor_reduce(
-                out=sums[hh][:],
-                in_=sbank[hh][:, 0 : 2 * P].rearrange("p (i u) -> p i u", u=2),
-                axis=mybir.AxisListType.X,
-                op=ADD,
+                out=sums[it][:], in_=sbank[it][:, 0 : 2 * P].rearrange("p (i u) -> p i u", u=2), axis=AXIS_X, op=ADD
             )
 
-        def relation_part(hh, engine):
-            it, h = hh // 2, hh % 2
-            if h == 0:
-                sgr[it] = work.tile([P, 1024], BF16, name="sgr", align_bytes=64)
+        def relation_part(it, b, engine):
+            if b == 0:
+                sgr[it] = two.tile([P, 1024], BF16, name="sgr", align_bytes=64)
             engine.tensor_tensor(
-                out=sgr[it][:, h * 512 : (h + 1) * 512].rearrange("p (i t) -> p i t", t=4),
-                in0=sums[hh][:].unsqueeze(2).to_broadcast([P, P, 4]),
-                in1=relf[:, h, :].unsqueeze(1).to_broadcast([P, P, 4]),
+                out=sgr[it][:, b * 512 : (b + 1) * 512].rearrange("p (i t) -> p i t", t=4),
+                in0=sums[it][:].unsqueeze(2).to_broadcast([P, P, 4]),
+                in1=relf[:, b * 4 : (b + 1) * 4].unsqueeze(1).to_broadcast([P, P, 4]),
                 op=MULT,
             )
 
-        def quantise_relation(it):
-            nc.vector.quantize_mx(
-                out=scodes[it][:, 4 * P : 6 * P].bitcast(FP8X4), scales=sscales[it][:, 4 * P : 6 * P], in_=sgr[it][:]
-            )
-
-        def quantise_nodes(hh, g0=0, n=2):
-            it, q0 = hh // 2, 2 * (hh % 2) + g0
-            if q0 == 0:
-                scodes[it] = four.tile([P, 6 * P], U32, name="scodes", align_bytes=64)
-                sscales[it] = four.tile([P, 6 * P], U8, name="sscales", align_bytes=64)
-            cols = slice(q0 * P, (q0 + n) * P)
+        def quantise_supports(it, j):
+            if it not in scodes:
+                scodes[it] = four.tile([P, PASSES * P], U32, name="scodes", align_bytes=64)
+                sscales[it] = four.tile([P, PASSES * P], U8, name="sscales", align_bytes=64)
+            cols = slice(j * 256, (j + 1) * 256)
             nc.vector.quantize_mx(
                 out=scodes[it][:, cols].bitcast(FP8X4),
                 scales=sscales[it][:, cols],
-                in_=sgn[it][:, q0 * 512 : (q0 + n) * 512],
+                in_=sgr[it][:] if j == 2 else sgn[it][:, j * 1024 : (j + 1) * 1024],
             )
 
         def project(it, passes):
             for q in passes:
-                if q == 0:
+                if q == 4:
                     obank[it] = ring.tile([P, 512], F32, name="bank")
                 nc.tensor.matmul_mx(
                     out=obank[it][:, 0:NB],
@@ -311,35 +323,42 @@ def tile_relationalgraphconvolution_pa_kernel(
                     lhsT_scale=sscales[it][:, q * P : (q + 1) * P],
                     rhs=w_codes[:, q * NB : (q + 1) * NB].bitcast(FP8X4),
                     rhs_scale=w_scales[:, q * NB : (q + 1) * NB],
-                    start=(q == 0),
+                    start=(q == 4),
                     stop=(q == 3),
                 )
 
         def store(it):
-            res = work.tile([P, NB], F32, name="res", align_bytes=64)
+            res = two.tile([P, NB], F32, name="res", align_bytes=64)
             nc.scalar.copy(out=res[:], in_=obank[it][:, 0:NB])
             nc.sync.dma_start(out=out[0, it * P : (it + 1) * P, :], in_=res[:])
 
-        def weight_values(pair, h):
-            c0 = h * R * F + pair * 1024
-            nc.vector.tensor_tensor(
-                out=w_val[:, c0 : c0 + 1024],
-                in0=w_bytes[:, c0 : c0 + 1024].bitcast(FP8),
-                in1=w_scale[:, pair * 1024 : (pair + 1) * 1024],
-                op=MULT,
+        def widen_weights(h, half):
+            r0 = half * R // 2
+            nc.vector.tensor_scalar(
+                out=w_val[h][:].rearrange("p (m r f) -> p r m f", r=R, f=16)[:, r0 : r0 + R // 2],
+                in0=w_bytes[h][:, r0 * F : (r0 + R // 2) * F].bitcast(FP8),
+                scalar1=one[:],
+                scalar2=None,
+                op0=MULT,
             )
 
         def turn_weights(q):
-            bank = ring.tile([P, 512], F32, name="bank")
-            words = w_val[:].bitcast(F32)
-            for h in range(2):
-                for u in range(2):
-                    k0 = (h * 2 + u) * P
-                    w0 = h * (R * F // 2) + q * 256
-                    nc.tensor.transpose(bank[:, k0 : k0 + P], words[:, w0 + u : w0 + 256 : 2], ident[:])
-            nc.scalar.copy(
-                out=w_grp[:, q * 1024 : (q + 1) * 1024].bitcast(F32).rearrange("p (h n u) -> p h n u", h=2, u=2),
-                in_=bank[:].rearrange("p (h u n) -> p h n u", h=2, u=2),
+            tbank[q] = ring.tile([P, 512], F32, name="bank")
+            for u in range(2):
+                for h in range(2):
+                    k0 = (u * 2 + h) * P
+                    w0 = (q * 2 + u) * P
+                    nc.tensor.transpose(tbank[q][:, k0 : k0 + P], w_val[h][:].bitcast(F32)[:, w0 : w0 + P], ident[:])
+
+        def scale_weights(q):
+            nc.vector.tensor_tensor(
+                out=w_grp[:, q * 1024 : (q + 1) * 1024].rearrange("p (n u e) -> p n u e", u=2, e=2),
+                in0=tbank[q][:].bitcast(BF16).rearrange("p (u n e) -> p n u e", u=2, e=2),
+                in1=w_scale[:, q * 4 : (q + 1) * 4]
+                .rearrange("p (u e) -> p u e", e=2)
+                .unsqueeze(1)
+                .to_broadcast([P, NB, 2, 2]),
+                op=MULT,
             )
 
         def quantise_weights(pair):
@@ -350,114 +369,123 @@ def tile_relationalgraphconvolution_pa_kernel(
                 in_=w_grp[:, pair * 2048 : (pair + 1) * 2048],
             )
 
-        all_passes = (0, 1, 4, 5, 2, 3)
+        all_passes = (4, 5, 0, 1, 2, 3)
         load(0, 4)
         load(1, 2)
         load_features()
         load(2, 2)
-        for s in range(3, PREFETCH):
+        load(3)
+        load_rows(rel_rows, relation_features[0])
+        load_rows(scale_rows, Wb_scale.rearrange("o (r f) -> (o r) f", f=F))
+        for s in range(4, PREFETCH):
             load(s)
-        nc.sync.dma_start(out=relf[:], in_=relation_features[0].rearrange("(h r) (q t) -> (r q) h t", h=2, t=4))
 
         project_at = {max(4 * it + PROJECT_LAG, 2 * it + FIRST_PROJECT): it for it in range(IT)}
 
-        def sort_step(s):
-            n = summed_on_vector(s)
-            for a in range(n):
-                sort_and_sum(s, a)
-            if s < 3:
-                for a in range(n, RG):
-                    sort(s, a, 1)
-            elif n < RG:
-                sort(s, n, RG - n)
-
-        def spread_half(hh):
-            n0, n1 = summed_on_vector(2 * hh), summed_on_vector(2 * hh + 1)
-            if n0 == n1:
-                spread_sums(2 * hh, 2)
-            else:
-                for s in (2 * hh, 2 * hh + 1):
-                    if summed_on_vector(s):
-                        spread_sums(s, 1)
-
         sort_step(0)
-        for s in range(STEPS - 1):
+        sort_step(1)
+        nc.vector.tensor_copy(
+            out=nf_grp[:].rearrange("p (c d t) -> p c d t", c=2, t=4),
+            in_=nf_raw[:].rearrange("p c (t d) -> p c d t", t=4),
+        )
+        for s in range(STEPS - 2):
             w = s - W0
-            if w + 4 in (0, 3, 6):
-                load_weights((w + 4) // 3)
+            it, phase = (s - 4) // GROUPS, s % GROUPS
+            if w + 3 in (0, 1):
+                nc.sync.dma_start(out=w_bytes[w + 3][:], in_=Wb_bytes[(w + 3) * P : (w + 4) * P, :])
             if s + PREFETCH < STEPS:
                 load(s + PREFETCH)
-            sort_step(s + 1)
+            if s >= 1:
+                quantise(s - 1)
+            if s == 1:
+                nc.vector.quantize_mx(out=nf_codes[:].bitcast(FP8X4), scales=nf_scales[:], in_=nf_grp[:])
+            if s == 3:
+                finish = [pick_own(relf, rel_rows, DR), pick_own(w_scale, scale_rows, F)]
+            if it >= 0 and phase == 2:
+                collect_sums(it)
+            if s + 2 < STEPS:
+                sort_step(s + 2)
+            if s == 3:
+                for reduce_picked in finish:
+                    reduce_picked()
+            if it >= 0 and phase >= 2:
+                relation_part(it, phase - 2, nc.vector)
             for a in range(RG):
                 empty(s, a, turn(s, a))
-            if s == 0:
-                nc.vector.tensor_copy(
-                    out=nf_grp[:].rearrange("p (c d t) -> p c d t", c=2, t=4),
-                    in_=nf_raw[:].rearrange("p c (t d) -> p c d t", t=4),
-                )
-                quantise(0)
-                nc.vector.quantize_mx(out=nf_codes[:].bitcast(FP8X4), scales=nf_scales[:], in_=nf_grp[:])
-            if s >= 3 and s % 2 == 1:
-                turn_sums((s - 3) // 2)
-            if s >= 4 and s % 2 == 0:
-                turn_supports((s - 4) // 2)
-            if 3 <= w < 15 and w % 4 in (3, 0):
-                turn_weights((w - 3) // 4 * 2 + (w - 3) % 4)
-            if 0 <= w < 12 and w % 2 == 0:
-                weight_values(w // 4, w // 2 % 2)
-            if 5 <= w < 17 and w % 4 == 1:
-                quantise_weights((w - 5) // 4)
-            if s >= 5 and s % 2 == 1:
-                quantise_nodes((s - 5) // 2)
-            if s >= 7 and s % 4 == 3:
-                quantise_relation((s - 7) // 4)
-            if s >= 1:
-                quantise(s)
-            if s >= 3 and s % 2 == 1:
-                collect_sums((s - 3) // 2)
-                relation_part((s - 3) // 2, nc.gpsimd)
-            if s == 1:
-                row_sums(0)
-                keep_sums(0)
-            if s >= 1:
-                aggregate(s - 1)
-                keep_supports(s - 1)
+            if it >= 0 and phase == 1:
+                turn_sums(it)
+            if it >= 0 and phase >= 2:
+                turn_supports(it, phase - 2)
+            if 5 <= w < 5 + PASSES:
+                turn_weights(w - 5)
+            if 0 <= w < 4:
+                widen_weights(w // 2, w % 2)
+            if w in (7, 9, 11):
+                quantise_weights((w - 7) // 2)
+            if it >= 0 and phase == 3:
+                quantise_supports(it, 0)
+            if it >= 1 and phase == 0:
+                quantise_supports(it - 1, 1)
+                quantise_supports(it - 1, 2)
+            if 5 <= w < 5 + PASSES:
+                scale_weights(w - 5)
+            if s >= 2:
+                aggregate(s - 2)
+                keep_supports(s - 2)
             if s in project_at:
                 project(project_at[s], all_passes)
                 store(project_at[s])
-            if s >= 2:
+            if s >= 1:
                 row_sums(s - 1)
-                keep_sums(s - 1)
-            if s % 2 == 1 and s > 1:
-                spread_half(s // 2)
+            if it >= 0 and phase == 0:
+                keep_sums(it)
+                spread_sums(it)
 
-        s, hh, it = STEPS - 1, HALVES - 1, IT - 1
+        s, it = STEPS - 2, IT - 1
+        quantise(s - 1)
+        collect_sums(it - 1)
+        for a in range(RG):
+            empty(s, a, turn(s, a))
+        for j in range(2):
+            relation_part(it - 1, j, nc.vector)
+            turn_supports(it - 1, j)
+        aggregate(s - 2)
+        keep_supports(s - 2)
+        project(it - 2, all_passes)
+        store(it - 2)
+        aggregate(s - 1)
+        keep_supports(s - 1)
+        quantise_supports(it - 1, 0)
+        quantise_supports(it - 1, 2)
+        quantise_supports(it - 1, 1)
         row_sums(s - 1)
-        keep_sums(s - 1)
-        spread_half(hh)
-        quantise_nodes(hh - 2)
-        quantise_relation(it - 1)
+
+        s = STEPS - 1
+        quantise(s - 1)
+        row_sums(s - 1)
+        keep_sums(it)
+        spread_sums(it)
         for a in range(RG):
             empty(s, a, turn(s, a), nc.vector.tensor_copy if a % 2 else nc.scalar.copy)
         quantise(s, 0, 2)
         quantise(s, 2, 2)
-        turn_sums(hh - 1)
-        collect_sums(hh - 1)
-        turn_supports(hh - 1)
-        turn_sums(hh)
+        turn_sums(it)
+        collect_sums(it)
         aggregate(s - 1)
         keep_supports(s - 1)
-        aggregate(s)
-        keep_supports(s)
-        collect_sums(hh)
-        relation_part(hh - 1, nc.vector)
-        quantise_nodes(hh - 1)
-        relation_part(hh, nc.vector)
         project(it - 1, all_passes)
-        turn_supports(hh)
+        aggregate(s, 0, 2)
+        keep_supports(s, 0, 2)
+        aggregate(s, 2, 2)
+        keep_supports(s, 2, 2)
+        relation_part(it, 0, nc.vector)
+        relation_part(it, 1, nc.vector)
+        turn_supports(it, 0)
+        quantise_supports(it, 2)
+        turn_supports(it, 1, nc.vector.tensor_copy)
         store(it - 1)
-        quantise_relation(it)
+        quantise_supports(it, 0)
         project(it, all_passes[:4])
-        quantise_nodes(hh)
+        quantise_supports(it, 1)
         project(it, all_passes[4:])
         store(it)

@@ -143,15 +143,18 @@ def tile_relationalgraphconvolution_pa_kernel(
             else:
                 dst = onep.tile([P, N], BF16, name="permone", align_bytes=64)
             for a in range(n):
-                perm[s, a0 + a] = (dst, n, a)
+                for c in range(2):
+                    h, k = divmod(2 * a + c, n)
+                    perm[s, a0 + a, c] = (dst, (2 * h * n + k) * P, n * P)
             nc.vector.tensor_copy(
-                out=dst[:].rearrange("p (u q f) -> p u q f", u=2, f=16),
-                in_=raw[s][:, a0 * N : (a0 + n) * N].rearrange("p (q u f) -> p u q f", u=2, f=16),
+                out=dst[:].rearrange("p (h u q f) -> p h u q f", h=2, u=2, f=16),
+                in_=raw[s][:, a0 * N : (a0 + n) * N].rearrange("p (h q u f) -> p h u q f", h=2, u=2, f=16),
             )
 
         def sort_and_sum(s, a):
             dst = onep.tile([P, N], BF16, name="permone", align_bytes=64)
-            perm[s, a] = (dst, 1, 0)
+            for c in range(2):
+                perm[s, a, c] = (dst, c * P, 2 * P)
             sorted_words = dst[:].rearrange("p (u q f) -> p u q f", u=2, f=16)
             row = raw[s][:, a * N : (a + 1) * N].rearrange("p (q u f) -> p u q f", u=2, f=16)
             total = rs[:, s * RG + a : s * RG + a + 1]
@@ -172,12 +175,12 @@ def tile_relationalgraphconvolution_pa_kernel(
         def turn(s, a):
             if a == 0:
                 grp[s] = three.tile([P, RG * N], BF16, name="grp", align_bytes=64)
-            src, n, al = perm[s, a]
             bank = ring.tile([P, 512], F32, name="bank")
             for c in range(2):
+                src, first, apart = perm[s, a, c]
                 for u in range(2):
                     k0 = (c * 2 + u) * P
-                    w0 = u * n * 256 + al * 256 + c * P
+                    w0 = first + u * apart
                     nc.tensor.transpose(bank[:, k0 : k0 + P], src[:].bitcast(F32)[:, w0 : w0 + P], ident[:])
             return bank
 

@@ -19,6 +19,7 @@ PASSES = F // 32
 PREFETCH = 5
 W0 = 3
 FIRST_PROJECT = W0 + 13
+CATCH_UP = 4
 PROJECT_LAG = 10
 
 F32 = mybir.dt.float32
@@ -36,6 +37,10 @@ FLOPS = 2 * (R * N * N * DE + N * R * F * NB)
 
 def summed_on_vector(s):
     return RG if s == STEPS - 1 else int(s >= FIRST_PROJECT)
+
+
+def sorted_on_scalar(s):
+    return int(W0 + 2 < s <= FIRST_PROJECT)
 
 
 def tile_relationalgraphconvolution_pa_kernel(
@@ -137,7 +142,7 @@ def tile_relationalgraphconvolution_pa_kernel(
                 op=ADD,
             )
 
-        def sort(s, a0, n):
+        def sort(s, a0, n, copy=nc.vector.tensor_copy):
             if n > 1:
                 dst = four.tile([P, n * N], BF16, name="perm", align_bytes=64)
             else:
@@ -146,7 +151,7 @@ def tile_relationalgraphconvolution_pa_kernel(
                 for c in range(2):
                     h, k = divmod(2 * a + c, n)
                     perm[s, a0 + a, c] = (dst, (2 * h * n + k) * P, n * P)
-            nc.vector.tensor_copy(
+            copy(
                 out=dst[:].rearrange("p (h u q f) -> p h u q f", h=2, u=2, f=16),
                 in_=raw[s][:, a0 * N : (a0 + n) * N].rearrange("p (h q u f) -> p h u q f", h=2, u=2, f=16),
             )
@@ -166,11 +171,11 @@ def tile_relationalgraphconvolution_pa_kernel(
             n = summed_on_vector(s)
             for a in range(summed_on_vector(s)):
                 sort_and_sum(s, a)
-            if s < 3:
+            if s <= 3:
                 for a in range(n, RG):
                     sort(s, a, 1)
             elif n < RG:
-                sort(s, n, RG - n)
+                sort(s, n, RG - n - sorted_on_scalar(s))
 
         def turn(s, a):
             if a == 0:
@@ -216,25 +221,25 @@ def tile_relationalgraphconvolution_pa_kernel(
                         stop=(c == 1),
                     )
 
-        def keep_supports(s, a0=0, n=RG):
+        def keep_supports(s, a0=0, n=RG, copy=nc.scalar.copy):
             it, r0 = s // GROUPS, s % GROUPS * RG + a0
             if r0 == 0:
                 supn[it] = two.tile([P, R * DE], BF16, name="supn", align_bytes=64)
-            nc.scalar.copy(
+            copy(
                 out=supn[it][:].rearrange("p (m r f) -> p m r f", r=R, f=16)[:, :, r0 : r0 + n, :],
                 in_=mx[s, a0][:, 0 : n * DE].rearrange("p (a m f) -> p m a f", a=n, f=16),
             )
 
-        def turn_supports(it, j, copy=nc.scalar.copy):
-            if j == 0:
+        def turn_supports(it, q0, n=2, copy=nc.scalar.copy):
+            if q0 == 0:
                 sgn[it] = two.tile([P, 2048], BF16, name="sgn", align_bytes=64)
             bank = ring.tile([P, 512], F32, name="bank")
-            for k in range(4):
-                w0 = (4 * j + k) * P
+            for k in range(2 * n):
+                w0 = (2 * q0 + k) * P
                 nc.tensor.transpose(bank[:, k * P : (k + 1) * P], supn[it][:].bitcast(F32)[:, w0 : w0 + P], ident[:])
             copy(
-                out=sgn[it][:, j * 1024 : (j + 1) * 1024].bitcast(F32).rearrange("p (b i u) -> p b i u", b=2, u=2),
-                in_=bank[:].rearrange("p (b u i) -> p b i u", b=2, u=2),
+                out=sgn[it][:, q0 * 512 : (q0 + n) * 512].bitcast(F32).rearrange("p (b i u) -> p b i u", b=n, u=2),
+                in_=bank[:, 0 : n * 256].rearrange("p (b u i) -> p b i u", b=n, u=2),
             )
 
         def row_sums(s):
@@ -305,15 +310,15 @@ def tile_relationalgraphconvolution_pa_kernel(
                 op=MULT,
             )
 
-        def quantise_supports(it, j):
+        def quantise_supports(it, q0, n=2):
             if it not in scodes:
                 scodes[it] = four.tile([P, PASSES * P], U32, name="scodes", align_bytes=64)
                 sscales[it] = four.tile([P, PASSES * P], U8, name="sscales", align_bytes=64)
-            cols = slice(j * 256, (j + 1) * 256)
+            cols = slice(q0 * P, (q0 + n) * P)
             nc.vector.quantize_mx(
                 out=scodes[it][:, cols].bitcast(FP8X4),
                 scales=sscales[it][:, cols],
-                in_=sgr[it][:] if j == 2 else sgn[it][:, j * 1024 : (j + 1) * 1024],
+                in_=sgr[it][:] if q0 == 4 else sgn[it][:, q0 * 512 : (q0 + n) * 512],
             )
 
         def project(it, passes):
@@ -377,7 +382,7 @@ def tile_relationalgraphconvolution_pa_kernel(
         load(1, 2)
         load_features()
         load(2, 2)
-        load(3)
+        load(3, 2)
         load_rows(rel_rows, relation_features[0])
         load_rows(scale_rows, Wb_scale.rearrange("o (r f) -> (o r) f", f=F))
         for s in range(4, PREFETCH):
@@ -406,7 +411,9 @@ def tile_relationalgraphconvolution_pa_kernel(
                 finish = [pick_own(relf, rel_rows, DR), pick_own(w_scale, scale_rows, F)]
             if it >= 0 and phase == 2:
                 collect_sums(it)
-            if s + 2 < STEPS:
+            if 1 <= s <= CATCH_UP:
+                sort_step(s + 1)
+            if CATCH_UP <= s < STEPS - 2:
                 sort_step(s + 2)
             if s == 3:
                 for reduce_picked in finish:
@@ -418,7 +425,7 @@ def tile_relationalgraphconvolution_pa_kernel(
             if it >= 0 and phase == 1:
                 turn_sums(it)
             if it >= 0 and phase >= 2:
-                turn_supports(it, phase - 2)
+                turn_supports(it, 2 * (phase - 2))
             if 5 <= w < 5 + PASSES:
                 turn_weights(w - 5)
             if 0 <= w < 4:
@@ -428,8 +435,8 @@ def tile_relationalgraphconvolution_pa_kernel(
             if it >= 0 and phase == 3:
                 quantise_supports(it, 0)
             if it >= 1 and phase == 0:
-                quantise_supports(it - 1, 1)
                 quantise_supports(it - 1, 2)
+                quantise_supports(it - 1, 4)
             if 5 <= w < 5 + PASSES:
                 scale_weights(w - 5)
             if s >= 2:
@@ -438,6 +445,8 @@ def tile_relationalgraphconvolution_pa_kernel(
             if s in project_at:
                 project(project_at[s], all_passes)
                 store(project_at[s])
+            if s + 2 < STEPS and sorted_on_scalar(s + 2):
+                sort(s + 2, RG - 1, 1, nc.scalar.copy)
             if s >= 1:
                 row_sums(s - 1)
             if it >= 0 and phase == 0:
@@ -451,7 +460,7 @@ def tile_relationalgraphconvolution_pa_kernel(
             empty(s, a, turn(s, a))
         for j in range(2):
             relation_part(it - 1, j, nc.vector)
-            turn_supports(it - 1, j)
+            turn_supports(it - 1, 2 * j)
         aggregate(s - 2)
         keep_supports(s - 2)
         project(it - 2, all_passes)
@@ -459,36 +468,35 @@ def tile_relationalgraphconvolution_pa_kernel(
         aggregate(s - 1)
         keep_supports(s - 1)
         quantise_supports(it - 1, 0)
+        quantise_supports(it - 1, 4)
         quantise_supports(it - 1, 2)
-        quantise_supports(it - 1, 1)
         row_sums(s - 1)
 
         s = STEPS - 1
         quantise(s - 1)
-        row_sums(s - 1)
-        keep_sums(it)
-        spread_sums(it)
         for a in range(RG):
             empty(s, a, turn(s, a), nc.vector.tensor_copy if a % 2 else nc.scalar.copy)
         quantise(s, 0, 2)
         quantise(s, 2, 2)
-        turn_sums(it)
-        collect_sums(it)
+        row_sums(s - 1)
+        keep_sums(it)
+        spread_sums(it)
         aggregate(s - 1)
         keep_supports(s - 1)
-        project(it - 1, all_passes)
+        turn_sums(it)
+        collect_sums(it)
         aggregate(s, 0, 2)
         keep_supports(s, 0, 2)
         aggregate(s, 2, 2)
         keep_supports(s, 2, 2)
         relation_part(it, 0, nc.vector)
         relation_part(it, 1, nc.vector)
-        turn_supports(it, 0)
-        quantise_supports(it, 2)
-        turn_supports(it, 1, nc.vector.tensor_copy)
+        project(it - 1, all_passes)
+        for q in range(4):
+            turn_supports(it, q, 1)
+        quantise_supports(it, 4)
+        for q in range(4):
+            quantise_supports(it, q, 1)
         store(it - 1)
-        quantise_supports(it, 0)
-        project(it, all_passes[:4])
-        quantise_supports(it, 1)
-        project(it, all_passes[4:])
+        project(it, all_passes)
         store(it)

@@ -18,8 +18,12 @@ GROUP = 8
 PASSES = F // 32
 PREFETCH = 5
 W0 = 3
-FIRST_PROJECT = W0 + 13
-CATCH_UP = 4
+W_WIDEN = 1
+W_GAP = 2
+FIRST_PROJECT = W0 + 3 * W_WIDEN + 2 + (PASSES - 1) * W_GAP + 3
+CATCH_UP = 5
+BAND_TILES = 8
+BAND_LAG = 3
 PROJECT_LAG = 10
 
 F32 = mybir.dt.float32
@@ -36,11 +40,19 @@ FLOPS = 2 * (R * N * N * DE + N * R * F * NB)
 
 
 def summed_on_vector(s):
-    return RG if s == STEPS - 1 else int(s >= FIRST_PROJECT)
+    return RG if s == STEPS - 1 else int(s >= FIRST_PROJECT - 1)
 
 
 def sorted_on_scalar(s):
-    return int(W0 + 2 < s <= FIRST_PROJECT)
+    return int(CATCH_UP + 1 < s <= FIRST_PROJECT and s % GROUPS != 2)
+
+
+def summed_by_band(s):
+    return min(max(BAND_TILES - RG * s, 0), RG)
+
+
+def not_narrow(s):
+    return summed_on_vector(s) + summed_by_band(s)
 
 
 def tile_relationalgraphconvolution_pa_kernel(
@@ -54,6 +66,7 @@ def tile_relationalgraphconvolution_pa_kernel(
         two = ctx.enter_context(tc.tile_pool(name="two", bufs=2))
         three = ctx.enter_context(tc.tile_pool(name="three", bufs=3))
         four = ctx.enter_context(tc.tile_pool(name="four", bufs=4))
+        many = ctx.enter_context(tc.tile_pool(name="many", bufs=5))
         ring = ctx.enter_context(tc.psum_pool(name="ring", bufs=6))
         sump = ctx.enter_context(tc.psum_pool(name="sump", bufs=1))
         ctx.enter_context(tc.manual_schedule())
@@ -61,7 +74,7 @@ def tile_relationalgraphconvolution_pa_kernel(
         ident = keep.tile([P, P], F32, name="ident", align_bytes=64)
         make_identity(nc, ident[:])
         rs = keep.tile([P, STEPS * RG], F32, name="rs", align_bytes=64)
-        patterns = [tuple(summed_on_vector(GROUPS * it + g) for g in range(GROUPS)) for it in range(IT)]
+        patterns = [tuple(not_narrow(GROUPS * it + g) for g in range(GROUPS)) for it in range(IT)]
         rep = {}
         for key in patterns:
             if key not in rep:
@@ -70,6 +83,9 @@ def tile_relationalgraphconvolution_pa_kernel(
                     nc.vector.memset(rep[key][:], 0.0)
         ones = keep.tile([P, GROUP], BF16, name="ones", align_bytes=64)
         nc.vector.memset(ones[:], 1.0)
+        band = keep.tile([P, 2 * P - GROUP], BF16, name="band", align_bytes=64)
+        nc.vector.memset(band[:], 0.0)
+        nc.vector.memset(band[:, P - GROUP : P], 1.0)
         one = keep.tile([P, 1], F32, name="one", align_bytes=64)
         nc.vector.memset(one[:], 1.0)
         pick = keep.tile([P, GROUP], F32, name="pick", align_bytes=64)
@@ -177,6 +193,19 @@ def tile_relationalgraphconvolution_pa_kernel(
             elif n < RG:
                 sort(s, n, RG - n - sorted_on_scalar(s))
 
+        def band_sum(r, c, u):
+            if 0 not in sbank:
+                sbank[0] = sump.tile([P, 512], F32, name="sbank")
+            c0 = r % RG * N + c * 512
+            words = grp[r // RG][:, c0 : c0 + 512].rearrange("p (i u e) -> p u i e", u=2, e=2)
+            nc.tensor.matmul(
+                sbank[0][:, 0 : 2 * P].rearrange("p (i e) -> p i e", e=2),
+                lhsT=band[:, P - GROUP * (r + 1) : 2 * P - GROUP * (r + 1)],
+                rhs=words[:, u],
+                start=(r == 0 and c == 0 and u == 0),
+                stop=False,
+            )
+
         def turn(s, a):
             if a == 0:
                 grp[s] = three.tile([P, RG * N], BF16, name="grp", align_bytes=64)
@@ -187,6 +216,8 @@ def tile_relationalgraphconvolution_pa_kernel(
                     k0 = (c * 2 + u) * P
                     w0 = first + u * apart
                     nc.tensor.transpose(bank[:, k0 : k0 + P], src[:].bitcast(F32)[:, w0 : w0 + P], ident[:])
+                    if 0 <= RG * s + a - BAND_LAG < BAND_TILES:
+                        band_sum(RG * s + a - BAND_LAG, c, u)
             return bank
 
         def empty(s, a, bank, copy=nc.scalar.copy):
@@ -242,12 +273,12 @@ def tile_relationalgraphconvolution_pa_kernel(
                 in_=bank[:, 0 : n * 256].rearrange("p (b u i) -> p b i u", b=n, u=2),
             )
 
-        def row_sums(s):
+        def row_sums(s, halves=(0, 1)):
             it, g = s // GROUPS, s % GROUPS
-            if g == 0:
+            if it not in wbank and not_narrow(s) < RG:
                 wbank[it] = sump.tile([P, 512], F32, name="wbank")
-            for a in range(summed_on_vector(s), RG):
-                for v in range(2):
+            for v in halves:
+                for a in range(not_narrow(s), RG):
                     k0 = v * P + (g * RG + a) * GROUP
                     for j in range(4):
                         c0 = a * N + j // 2 * 512 + v * 256
@@ -282,14 +313,15 @@ def tile_relationalgraphconvolution_pa_kernel(
                     )
 
         def turn_sums(it):
-            sbank[it] = sump.tile([P, 512], F32, name="sbank")
-            parts = 3 if sum(patterns[it]) else 2
+            if it > 0:
+                sbank[it] = sump.tile([P, 512], F32, name="sbank")
+            parts = 3 if it > 0 and sum(patterns[it]) else 2
             for v in range(parts):
                 nc.tensor.matmul(
                     sbank[it][:, v * P : (v + 1) * P] if v < 2 else sbank[it][:, 0 : 2 * P : 2],
                     lhsT=rep[patterns[it]][:, v * P : (v + 1) * P],
                     rhs=ident[:],
-                    start=(v == 0),
+                    start=(v == 0 and it > 0),
                     stop=(v == parts - 1),
                     is_transpose=True,
                 )
@@ -312,8 +344,8 @@ def tile_relationalgraphconvolution_pa_kernel(
 
         def quantise_supports(it, q0, n=2):
             if it not in scodes:
-                scodes[it] = four.tile([P, PASSES * P], U32, name="scodes", align_bytes=64)
-                sscales[it] = four.tile([P, PASSES * P], U8, name="sscales", align_bytes=64)
+                scodes[it] = many.tile([P, PASSES * P], U32, name="scodes", align_bytes=64)
+                sscales[it] = many.tile([P, PASSES * P], U8, name="sscales", align_bytes=64)
             cols = slice(q0 * P, (q0 + n) * P)
             nc.vector.quantize_mx(
                 out=scodes[it][:, cols].bitcast(FP8X4),
@@ -398,6 +430,7 @@ def tile_relationalgraphconvolution_pa_kernel(
         )
         for s in range(STEPS - 2):
             w = s - W0
+            wt = w - 3 * W_WIDEN - 2
             it, phase = (s - 4) // GROUPS, s % GROUPS
             if w + 3 in (0, 1):
                 nc.sync.dma_start(out=w_bytes[w + 3][:], in_=Wb_bytes[(w + 3) * P : (w + 4) * P, :])
@@ -426,19 +459,21 @@ def tile_relationalgraphconvolution_pa_kernel(
                 turn_sums(it)
             if it >= 0 and phase >= 2:
                 turn_supports(it, 2 * (phase - 2))
-            if 5 <= w < 5 + PASSES:
-                turn_weights(w - 5)
-            if 0 <= w < 4:
-                widen_weights(w // 2, w % 2)
-            if w in (7, 9, 11):
-                quantise_weights((w - 7) // 2)
+            if 0 <= wt < W_GAP * PASSES and wt % W_GAP == 0:
+                turn_weights(wt // W_GAP)
+            if 0 <= w < 4 * W_WIDEN and w % W_WIDEN == 0:
+                widen_weights(w // W_WIDEN // 2, w // W_WIDEN % 2)
+            if 0 < wt <= W_GAP * PASSES and (wt - 1) % (2 * W_GAP) == W_GAP:
+                quantise_weights((wt - 1) // (2 * W_GAP))
             if it >= 0 and phase == 3:
                 quantise_supports(it, 0)
             if it >= 1 and phase == 0:
                 quantise_supports(it - 1, 2)
                 quantise_supports(it - 1, 4)
-            if 5 <= w < 5 + PASSES:
-                scale_weights(w - 5)
+            if 0 <= wt < W_GAP * PASSES and wt % W_GAP == 0:
+                scale_weights(wt // W_GAP)
+            if s >= 1:
+                row_sums(s - 1, (0,))
             if s >= 2:
                 aggregate(s - 2)
                 keep_supports(s - 2)
@@ -448,9 +483,10 @@ def tile_relationalgraphconvolution_pa_kernel(
             if s + 2 < STEPS and sorted_on_scalar(s + 2):
                 sort(s + 2, RG - 1, 1, nc.scalar.copy)
             if s >= 1:
-                row_sums(s - 1)
+                row_sums(s - 1, (1,))
             if it >= 0 and phase == 0:
                 keep_sums(it)
+            if it >= 1 and phase == 0:
                 spread_sums(it)
 
         s, it = STEPS - 2, IT - 1

@@ -17,13 +17,14 @@ STEPS = IT * GROUPS
 GROUP = 8
 PASSES = F // 32
 PREFETCH = 5
-W0 = 3
-W_WIDEN = 1
-W_GAP = 2
-FIRST_PROJECT = W0 + 3 * W_WIDEN + 2 + (PASSES - 1) * W_GAP + 3
-CATCH_UP = 5
+W0 = 4
+W_TURN = 9
+FIRST_PROJECT = 22
+CATCH_UP = 6
 BAND_TILES = 8
 BAND_LAG = 3
+W_LOAD = 1
+HALVED = 7
 PROJECT_LAG = 10
 
 F32 = mybir.dt.float32
@@ -40,11 +41,11 @@ FLOPS = 2 * (R * N * N * DE + N * R * F * NB)
 
 
 def summed_on_vector(s):
-    return RG if s == STEPS - 1 else int(s >= FIRST_PROJECT - 1)
+    return RG if s == STEPS - 1 else int(s >= FIRST_PROJECT)
 
 
 def sorted_on_scalar(s):
-    return int(CATCH_UP + 1 < s <= FIRST_PROJECT and s % GROUPS != 2)
+    return int(W_TURN + 1 < s < STEPS - 1 and s % GROUPS == 3)
 
 
 def summed_by_band(s):
@@ -121,7 +122,6 @@ def tile_relationalgraphconvolution_pa_kernel(
         scodes = {}
         sscales = {}
         obank = {}
-        tbank = {}
 
         def load(s, pieces=1):
             it, g = s // GROUPS, s % GROUPS
@@ -190,6 +190,9 @@ def tile_relationalgraphconvolution_pa_kernel(
             if s <= 3:
                 for a in range(n, RG):
                     sort(s, a, 1)
+            elif s <= HALVED:
+                sort(s, 0, 2)
+                sort(s, 2, 2 - sorted_on_scalar(s))
             elif n < RG:
                 sort(s, n, RG - n - sorted_on_scalar(s))
 
@@ -383,21 +386,23 @@ def tile_relationalgraphconvolution_pa_kernel(
             )
 
         def turn_weights(q):
-            tbank[q] = ring.tile([P, 512], F32, name="bank")
+            bank = ring.tile([P, 512], F32, name="bank")
             for u in range(2):
                 for h in range(2):
                     k0 = (u * 2 + h) * P
                     w0 = (q * 2 + u) * P
-                    nc.tensor.transpose(tbank[q][:, k0 : k0 + P], w_val[h][:].bitcast(F32)[:, w0 : w0 + P], ident[:])
+                    nc.tensor.transpose(bank[:, k0 : k0 + P], w_val[h][:].bitcast(F32)[:, w0 : w0 + P], ident[:])
+            nc.scalar.copy(
+                out=w_grp[:, q * 1024 : (q + 1) * 1024].bitcast(F32).rearrange("p (n u) -> p n u", u=2),
+                in_=bank[:].rearrange("p (u n) -> p n u", u=2),
+            )
 
         def scale_weights(q):
+            values = w_grp[:, q * 1024 : (q + 1) * 1024].rearrange("p (n t) -> p n t", t=4)
             nc.vector.tensor_tensor(
-                out=w_grp[:, q * 1024 : (q + 1) * 1024].rearrange("p (n u e) -> p n u e", u=2, e=2),
-                in0=tbank[q][:].bitcast(BF16).rearrange("p (u n e) -> p n u e", u=2, e=2),
-                in1=w_scale[:, q * 4 : (q + 1) * 4]
-                .rearrange("p (u e) -> p u e", e=2)
-                .unsqueeze(1)
-                .to_broadcast([P, NB, 2, 2]),
+                out=values,
+                in0=values,
+                in1=w_scale[:, q * 4 : (q + 1) * 4].unsqueeze(1).to_broadcast([P, NB, 4]),
                 op=MULT,
             )
 
@@ -418,9 +423,9 @@ def tile_relationalgraphconvolution_pa_kernel(
         load_rows(rel_rows, relation_features[0])
         load_rows(scale_rows, Wb_scale.rearrange("o (r f) -> (o r) f", f=F))
         for s in range(4, PREFETCH):
-            load(s)
+            load(s, 2 if s <= HALVED else 1)
 
-        project_at = {max(4 * it + PROJECT_LAG, 2 * it + FIRST_PROJECT): it for it in range(IT)}
+        project_at = {max(4 * it + PROJECT_LAG, 3 * it // 2 + FIRST_PROJECT): it for it in range(IT)}
 
         sort_step(0)
         sort_step(1)
@@ -430,19 +435,21 @@ def tile_relationalgraphconvolution_pa_kernel(
         )
         for s in range(STEPS - 2):
             w = s - W0
-            wt = w - 3 * W_WIDEN - 2
             it, phase = (s - 4) // GROUPS, s % GROUPS
-            if w + 3 in (0, 1):
-                nc.sync.dma_start(out=w_bytes[w + 3][:], in_=Wb_bytes[(w + 3) * P : (w + 4) * P, :])
+            pair, stage = divmod(s - W_TURN, GROUPS)
+            weights = 0 <= pair < PASSES // 2
+            h = s - W_LOAD
+            if h in (0, 1):
+                nc.sync.dma_start(out=w_bytes[h][:], in_=Wb_bytes[h * P : (h + 1) * P, :])
             if s + PREFETCH < STEPS:
-                load(s + PREFETCH)
+                load(s + PREFETCH, 2 if s + PREFETCH <= HALVED else 1)
             if s >= 1:
                 quantise(s - 1)
             if s == 1:
                 nc.vector.quantize_mx(out=nf_codes[:].bitcast(FP8X4), scales=nf_scales[:], in_=nf_grp[:])
             if s == 3:
                 finish = [pick_own(relf, rel_rows, DR), pick_own(w_scale, scale_rows, F)]
-            if it >= 0 and phase == 2:
+            if it >= 0 and phase == 3:
                 collect_sums(it)
             if 1 <= s <= CATCH_UP:
                 sort_step(s + 1)
@@ -451,28 +458,29 @@ def tile_relationalgraphconvolution_pa_kernel(
             if s == 3:
                 for reduce_picked in finish:
                     reduce_picked()
-            if it >= 0 and phase >= 2:
-                relation_part(it, phase - 2, nc.vector)
             for a in range(RG):
                 empty(s, a, turn(s, a))
-            if it >= 0 and phase == 1:
+            if it >= 0 and phase == 2:
                 turn_sums(it)
             if it >= 0 and phase >= 2:
                 turn_supports(it, 2 * (phase - 2))
-            if 0 <= wt < W_GAP * PASSES and wt % W_GAP == 0:
-                turn_weights(wt // W_GAP)
-            if 0 <= w < 4 * W_WIDEN and w % W_WIDEN == 0:
-                widen_weights(w // W_WIDEN // 2, w // W_WIDEN % 2)
-            if 0 < wt <= W_GAP * PASSES and (wt - 1) % (2 * W_GAP) == W_GAP:
-                quantise_weights((wt - 1) // (2 * W_GAP))
+            if weights and stage < 2:
+                turn_weights(2 * pair + stage)
+            if weights and stage in (1, 2):
+                scale_weights(2 * pair + stage - 1)
+            if 0 <= w < 4:
+                widen_weights(w // 2, w % 2)
+            if weights and stage == 3:
+                quantise_weights(pair)
             if it >= 0 and phase == 3:
+                relation_part(it, 0, nc.vector)
                 quantise_supports(it, 0)
             if it >= 1 and phase == 0:
+                relation_part(it - 1, 1, nc.vector)
                 quantise_supports(it - 1, 2)
+            if it >= 1 and phase == 1:
                 quantise_supports(it - 1, 4)
-            if 0 <= wt < W_GAP * PASSES and wt % W_GAP == 0:
-                scale_weights(wt // W_GAP)
-            if s >= 1:
+            if s >= 1 and phase != 1:
                 row_sums(s - 1, (0,))
             if s >= 2:
                 aggregate(s - 2)
@@ -483,55 +491,50 @@ def tile_relationalgraphconvolution_pa_kernel(
             if s + 2 < STEPS and sorted_on_scalar(s + 2):
                 sort(s + 2, RG - 1, 1, nc.scalar.copy)
             if s >= 1:
-                row_sums(s - 1, (1,))
+                row_sums(s - 1, (0, 1) if phase == 1 else (1,))
             if it >= 0 and phase == 0:
                 keep_sums(it)
             if it >= 1 and phase == 0:
                 spread_sums(it)
 
-        s, it = STEPS - 2, IT - 1
-        quantise(s - 1)
+        s, it = STEPS - 1, IT - 1
+        quantise(s - 2)
+        for a in range(RG):
+            empty(s - 1, a, turn(s - 1, a))
+        turn_sums(it - 1)
         collect_sums(it - 1)
         for a in range(RG):
-            empty(s, a, turn(s, a))
-        for j in range(2):
-            relation_part(it - 1, j, nc.vector)
-            turn_supports(it - 1, 2 * j)
-        aggregate(s - 2)
-        keep_supports(s - 2)
-        project(it - 2, all_passes)
-        store(it - 2)
-        aggregate(s - 1)
-        keep_supports(s - 1)
-        quantise_supports(it - 1, 0)
-        quantise_supports(it - 1, 4)
-        quantise_supports(it - 1, 2)
-        row_sums(s - 1)
-
-        s = STEPS - 1
+            empty(s, a, turn(s, a), nc.scalar.copy if a % 2 else nc.vector.tensor_copy)
         quantise(s - 1)
-        for a in range(RG):
-            empty(s, a, turn(s, a), nc.vector.tensor_copy if a % 2 else nc.scalar.copy)
-        quantise(s, 0, 2)
-        quantise(s, 2, 2)
+        quantise(s)
+        for j in range(2):
+            turn_supports(it - 1, 2 * j)
+            relation_part(it - 1, j, nc.vector)
+        row_sums(s - 2)
+        for k in (s - 3, s - 2):
+            aggregate(k)
+            keep_supports(k)
         row_sums(s - 1)
         keep_sums(it)
         spread_sums(it)
-        aggregate(s - 1)
-        keep_supports(s - 1)
+        for k in (s - 1, s):
+            aggregate(k)
+            keep_supports(k)
+        quantise_supports(it - 1, 0)
+        quantise_supports(it - 1, 4)
+        quantise_supports(it - 1, 2)
         turn_sums(it)
+        project(it - 2, all_passes)
         collect_sums(it)
-        aggregate(s, 0, 2)
-        keep_supports(s, 0, 2)
-        aggregate(s, 2, 2)
-        keep_supports(s, 2, 2)
         relation_part(it, 0, nc.vector)
         relation_part(it, 1, nc.vector)
-        project(it - 1, all_passes)
+        store(it - 2)
         for q in range(4):
             turn_supports(it, q, 1)
+        project(it - 1, all_passes)
+        quantise_supports(it, 0, 1)
         quantise_supports(it, 4)
-        for q in range(4):
+        for q in range(1, 4):
             quantise_supports(it, q, 1)
         store(it - 1)
         project(it, all_passes)

@@ -20,11 +20,11 @@ PREFETCH = 5
 W0 = 4
 W_TURN = 9
 FIRST_PROJECT = 22
-CATCH_UP = 6
-BAND_TILES = 8
+CATCH_UP = 7
+BAND_TILES = 4
 BAND_LAG = 3
 W_LOAD = 1
-HALVED = 7
+HALVED = 8
 PROJECT_LAG = 10
 
 F32 = mybir.dt.float32
@@ -45,7 +45,7 @@ def summed_on_vector(s):
 
 
 def sorted_on_scalar(s):
-    return int(W_TURN + 1 < s < STEPS - 1 and s % GROUPS == 3)
+    return int(W_TURN + 1 < s < STEPS - 1 and s % (2 if s < FIRST_PROJECT else GROUPS) == (1 if s < FIRST_PROJECT else 3))
 
 
 def summed_by_band(s):
@@ -219,8 +219,9 @@ def tile_relationalgraphconvolution_pa_kernel(
                     k0 = (c * 2 + u) * P
                     w0 = first + u * apart
                     nc.tensor.transpose(bank[:, k0 : k0 + P], src[:].bitcast(F32)[:, w0 : w0 + P], ident[:])
-                    if 0 <= RG * s + a - BAND_LAG < BAND_TILES:
-                        band_sum(RG * s + a - BAND_LAG, c, u)
+            if 0 <= RG * s + a - BAND_LAG < BAND_TILES:
+                for k in range(4):
+                    band_sum(RG * s + a - BAND_LAG, k // 2, k % 2)
             return bank
 
         def empty(s, a, bank, copy=nc.scalar.copy):
@@ -417,8 +418,8 @@ def tile_relationalgraphconvolution_pa_kernel(
         all_passes = (4, 5, 0, 1, 2, 3)
         load(0, 4)
         load(1, 2)
-        load_features()
         load(2, 2)
+        load_features()
         load(3, 2)
         load_rows(rel_rows, relation_features[0])
         load_rows(scale_rows, Wb_scale.rearrange("o (r f) -> (o r) f", f=F))
@@ -429,10 +430,6 @@ def tile_relationalgraphconvolution_pa_kernel(
 
         sort_step(0)
         sort_step(1)
-        nc.vector.tensor_copy(
-            out=nf_grp[:].rearrange("p (c d t) -> p c d t", c=2, t=4),
-            in_=nf_raw[:].rearrange("p c (t d) -> p c d t", t=4),
-        )
         for s in range(STEPS - 2):
             w = s - W0
             it, phase = (s - 4) // GROUPS, s % GROUPS
@@ -443,16 +440,21 @@ def tile_relationalgraphconvolution_pa_kernel(
                 nc.sync.dma_start(out=w_bytes[h][:], in_=Wb_bytes[h * P : (h + 1) * P, :])
             if s + PREFETCH < STEPS:
                 load(s + PREFETCH, 2 if s + PREFETCH <= HALVED else 1)
+            if s == 2:
+                nc.vector.quantize_mx(out=nf_codes[:].bitcast(FP8X4), scales=nf_scales[:], in_=nf_grp[:])
             if s >= 1:
                 quantise(s - 1)
-            if s == 1:
-                nc.vector.quantize_mx(out=nf_codes[:].bitcast(FP8X4), scales=nf_scales[:], in_=nf_grp[:])
             if s == 3:
                 finish = [pick_own(relf, rel_rows, DR), pick_own(w_scale, scale_rows, F)]
             if it >= 0 and phase == 3:
                 collect_sums(it)
             if 1 <= s <= CATCH_UP:
                 sort_step(s + 1)
+            if s == 1:
+                nc.vector.tensor_copy(
+                    out=nf_grp[:].rearrange("p (c d t) -> p c d t", c=2, t=4),
+                    in_=nf_raw[:].rearrange("p c (t d) -> p c d t", t=4),
+                )
             if CATCH_UP <= s < STEPS - 2:
                 sort_step(s + 2)
             if s == 3:
@@ -481,7 +483,7 @@ def tile_relationalgraphconvolution_pa_kernel(
             if it >= 1 and phase == 1:
                 quantise_supports(it - 1, 4)
             if s >= 1 and phase != 1:
-                row_sums(s - 1, (0,))
+                row_sums(s - 1, (0, 1) if s == 2 else (0,))
             if s >= 2:
                 aggregate(s - 2)
                 keep_supports(s - 2)
@@ -490,7 +492,7 @@ def tile_relationalgraphconvolution_pa_kernel(
                 store(project_at[s])
             if s + 2 < STEPS and sorted_on_scalar(s + 2):
                 sort(s + 2, RG - 1, 1, nc.scalar.copy)
-            if s >= 1:
+            if s >= 1 and s != 2:
                 row_sums(s - 1, (0, 1) if phase == 1 else (1,))
             if it >= 0 and phase == 0:
                 keep_sums(it)

@@ -20,11 +20,13 @@ PREFETCH = 5
 W0 = 4
 W_TURN = 9
 FIRST_PROJECT = 22
-CATCH_UP = 7
+CATCH_UP = 8
 BAND_TILES = 4
 BAND_LAG = 3
 W_LOAD = 1
-HALVED = 8
+HALVED = 9
+ROWS_LOAD = 0
+ROWS_PICK = 5
 PROJECT_LAG = 10
 
 F32 = mybir.dt.float32
@@ -41,11 +43,11 @@ FLOPS = 2 * (R * N * N * DE + N * R * F * NB)
 
 
 def summed_on_vector(s):
-    return RG if s == STEPS - 1 else int(s >= FIRST_PROJECT)
+    return RG if s == STEPS - 1 else int(s > FIRST_PROJECT)
 
 
 def sorted_on_scalar(s):
-    return int(W_TURN + 1 < s < STEPS - 1 and s % (2 if s < FIRST_PROJECT else GROUPS) == (1 if s < FIRST_PROJECT else 3))
+    return int(CATCH_UP + 2 < s < STEPS - 1 and s % GROUPS == GROUPS - 1)
 
 
 def summed_by_band(s):
@@ -79,7 +81,8 @@ def tile_relationalgraphconvolution_pa_kernel(
         rep = {}
         for key in patterns:
             if key not in rep:
-                rep[key] = keep.tile([P, 3 * P], F32, name="rep%d%d%d%d" % key, align_bytes=64)
+                parts = 2 if key == patterns[0] or not sum(key) else 3
+                rep[key] = keep.tile([P, parts * P], F32, name="rep%d%d%d%d" % key, align_bytes=64)
                 if sum(key):
                     nc.vector.memset(rep[key][:], 0.0)
         ones = keep.tile([P, GROUP], BF16, name="ones", align_bytes=64)
@@ -421,8 +424,6 @@ def tile_relationalgraphconvolution_pa_kernel(
         load(2, 2)
         load_features()
         load(3, 2)
-        load_rows(rel_rows, relation_features[0])
-        load_rows(scale_rows, Wb_scale.rearrange("o (r f) -> (o r) f", f=F))
         for s in range(4, PREFETCH):
             load(s, 2 if s <= HALVED else 1)
 
@@ -440,11 +441,14 @@ def tile_relationalgraphconvolution_pa_kernel(
                 nc.sync.dma_start(out=w_bytes[h][:], in_=Wb_bytes[h * P : (h + 1) * P, :])
             if s + PREFETCH < STEPS:
                 load(s + PREFETCH, 2 if s + PREFETCH <= HALVED else 1)
+            if s == ROWS_LOAD:
+                load_rows(rel_rows, relation_features[0])
+                load_rows(scale_rows, Wb_scale.rearrange("o (r f) -> (o r) f", f=F))
             if s == 2:
                 nc.vector.quantize_mx(out=nf_codes[:].bitcast(FP8X4), scales=nf_scales[:], in_=nf_grp[:])
             if s >= 1:
                 quantise(s - 1)
-            if s == 3:
+            if s == ROWS_PICK:
                 finish = [pick_own(relf, rel_rows, DR), pick_own(w_scale, scale_rows, F)]
             if it >= 0 and phase == 3:
                 collect_sums(it)
@@ -457,7 +461,7 @@ def tile_relationalgraphconvolution_pa_kernel(
                 )
             if CATCH_UP <= s < STEPS - 2:
                 sort_step(s + 2)
-            if s == 3:
+            if s == ROWS_PICK:
                 for reduce_picked in finish:
                     reduce_picked()
             for a in range(RG):
@@ -496,7 +500,7 @@ def tile_relationalgraphconvolution_pa_kernel(
                 row_sums(s - 1, (0, 1) if phase == 1 else (1,))
             if it >= 0 and phase == 0:
                 keep_sums(it)
-            if it >= 1 and phase == 0:
+            if it >= 1 and phase == 0 and sum(patterns[it]):
                 spread_sums(it)
 
         s, it = STEPS - 1, IT - 1

@@ -20,13 +20,14 @@ PREFETCH = 5
 W0 = 4
 W_TURN = 9
 FIRST_PROJECT = 22
-CATCH_UP = 8
+CATCH_UP = 7
 BAND_TILES = 4
 BAND_LAG = 3
 W_LOAD = 1
-HALVED = 9
+HALVED = 8
 ROWS_LOAD = 0
 ROWS_PICK = 5
+REGROUP = 3
 PROJECT_LAG = 10
 
 F32 = mybir.dt.float32
@@ -43,11 +44,7 @@ FLOPS = 2 * (R * N * N * DE + N * R * F * NB)
 
 
 def summed_on_vector(s):
-    return RG if s == STEPS - 1 else int(s > FIRST_PROJECT)
-
-
-def sorted_on_scalar(s):
-    return int(CATCH_UP + 2 < s < STEPS - 1 and s % GROUPS == GROUPS - 1)
+    return RG if s == STEPS - 1 else int(s >= FIRST_PROJECT - 1)
 
 
 def summed_by_band(s):
@@ -64,11 +61,11 @@ def tile_relationalgraphconvolution_pa_kernel(
     nc = tc.nc
     with ExitStack() as ctx:
         keep = ctx.enter_context(tc.tile_pool(name="keep", bufs=1))
-        rawp = ctx.enter_context(tc.tile_pool(name="rawp", bufs=PREFETCH + 1))
+        rawp = ctx.enter_context(tc.tile_pool(name="rawp", bufs=PREFETCH + 3))
         onep = ctx.enter_context(tc.tile_pool(name="onep", bufs=8))
         two = ctx.enter_context(tc.tile_pool(name="two", bufs=2))
         three = ctx.enter_context(tc.tile_pool(name="three", bufs=3))
-        four = ctx.enter_context(tc.tile_pool(name="four", bufs=4))
+        four = ctx.enter_context(tc.tile_pool(name="four", bufs=5))
         many = ctx.enter_context(tc.tile_pool(name="many", bufs=5))
         ring = ctx.enter_context(tc.psum_pool(name="ring", bufs=6))
         sump = ctx.enter_context(tc.psum_pool(name="sump", bufs=1))
@@ -96,10 +93,15 @@ def tile_relationalgraphconvolution_pa_kernel(
         nc.vector.tensor_reduce(
             out=pick[:], in_=ident[:].rearrange("p (g x) -> p x g", x=GROUP), axis=AXIS_X, op=ADD
         )
+        regroup = keep.tile([P, P], BF16, name="regroup", align_bytes=64)
+        nc.vector.tensor_copy(
+            out=regroup[:].rearrange("p (j h x) -> p j h x", h=2, x=GROUP),
+            in_=ident[:].rearrange("p (h j x) -> p j h x", h=2, x=GROUP),
+        )
         nf_raw = keep.tile([P, 2, 4 * DE], BF16, name="nf_raw", align_bytes=64)
-        nf_grp = keep.tile([P, 2 * 4 * DE], BF16, name="nf_grp", align_bytes=64)
-        nf_codes = keep.tile([P, 2 * DE], U32, name="nf_codes", align_bytes=64)
-        nf_scales = keep.tile([P, 2 * DE], U8, name="nf_scales", align_bytes=64)
+        nf_grp = keep.tile([P, 4 * 4 * DE], BF16, name="nf_grp", align_bytes=64)
+        nf_codes = keep.tile([P, 4 * DE], U32, name="nf_codes", align_bytes=64)
+        nf_scales = keep.tile([P, 4 * DE], U8, name="nf_scales", align_bytes=64)
         rel_rows = keep.tile([P, DR], BF16, name="rel_rows", align_bytes=64)
         relf = keep.tile([P, 2 * 4], F32, name="relf", align_bytes=64)
         scale_rows = keep.tile([P, F], F32, name="scale_rows", align_bytes=64)
@@ -143,6 +145,23 @@ def tile_relationalgraphconvolution_pa_kernel(
                 for u in range(2):
                     nc.sync.dma_start(out=nf_raw[:, c, u * 2 * DE : (u + 1) * 2 * DE], in_=runs[c, u])
 
+        def regroup_features():
+            for c in range(2):
+                bank = ring.tile([P, 512], F32, name="bank")
+                nc.tensor.matmul(bank[:], lhsT=regroup[:], rhs=nf_raw[:, c, :], start=True, stop=True)
+                nc.scalar.copy(
+                    out=nf_grp[:, 1024 + c * 512 : 1024 + (c + 1) * 512].rearrange("p (d t) -> p d t", t=4),
+                    in_=bank[:].rearrange("p (t d) -> p d t", t=4),
+                )
+
+        def quantise_features(v):
+            cols = slice(v * 256, (v + 1) * 256)
+            nc.vector.quantize_mx(
+                out=nf_codes[:, cols].bitcast(FP8X4),
+                scales=nf_scales[:, cols],
+                in_=nf_grp[:, v * 1024 : (v + 1) * 1024],
+            )
+
         def load_rows(dst, rows):
             nc.sync.dma_start(out=dst[:], in_=rows.partition_broadcast(GROUP).rearrange("x r f -> r x f"))
 
@@ -161,24 +180,38 @@ def tile_relationalgraphconvolution_pa_kernel(
                 op=ADD,
             )
 
-        def sort(s, a0, n, copy=nc.vector.tensor_copy):
-            if n > 1:
-                dst = four.tile([P, n * N], BF16, name="perm", align_bytes=64)
-            else:
-                dst = onep.tile([P, N], BF16, name="permone", align_bytes=64)
+        def sort(s, a0, n):
+            dst = onep.tile([P, N], BF16, name="permone", align_bytes=64)
             for a in range(n):
                 for c in range(2):
                     h, k = divmod(2 * a + c, n)
-                    perm[s, a0 + a, c] = (dst, (2 * h * n + k) * P, n * P)
-            copy(
+                    perm[s, a0 + a, c] = [(dst, ((2 * h + u) * n + k) * P) for u in range(2)]
+            nc.vector.tensor_copy(
                 out=dst[:].rearrange("p (h u q f) -> p h u q f", h=2, u=2, f=16),
                 in_=raw[s][:, a0 * N : (a0 + n) * N].rearrange("p (h q u f) -> p h u q f", h=2, u=2, f=16),
             )
 
+        def exchanged(s):
+            return range(summed_on_vector(s), RG) if s > 3 else range(0)
+
+        def gather_seconds(s, tiles):
+            dst = four.tile([P, len(tiles) * 512], BF16, name="seconds", align_bytes=64)
+            for a in tiles:
+                for c in range(2):
+                    perm[s, a, c] = ((raw[s], (4 * a + 2 * c) * P), (dst, (2 * (a - tiles[0]) + c) * P))
+            rows = raw[s][:, tiles[0] * N : (tiles[-1] + 1) * N].rearrange("p (m h j u f) -> p m h j u f", h=2, j=8, u=2, f=16)
+            nc.vector.tensor_copy(
+                out=dst[:].rearrange("p (m j h f) -> p m h j f", j=8, h=2, f=16), in_=rows[:, :, :, :, 1, :]
+            )
+
+        def gather_firsts(s, tiles):
+            rows = raw[s][:, tiles[0] * N : (tiles[-1] + 1) * N].rearrange("p (m h j u f) -> p m h j u f", h=2, j=8, u=2, f=16)
+            nc.vector.tensor_copy(out=rows[:, :, 0, :, 1, :], in_=rows[:, :, 1, :, 0, :])
+
         def sort_and_sum(s, a):
             dst = onep.tile([P, N], BF16, name="permone", align_bytes=64)
             for c in range(2):
-                perm[s, a, c] = (dst, c * P, 2 * P)
+                perm[s, a, c] = [(dst, (2 * u + c) * P) for u in range(2)]
             sorted_words = dst[:].rearrange("p (u q f) -> p u q f", u=2, f=16)
             row = raw[s][:, a * N : (a + 1) * N].rearrange("p (q u f) -> p u q f", u=2, f=16)
             total = rs[:, s * RG + a : s * RG + a + 1]
@@ -194,10 +227,11 @@ def tile_relationalgraphconvolution_pa_kernel(
                 for a in range(n, RG):
                     sort(s, a, 1)
             elif s <= HALVED:
-                sort(s, 0, 2)
-                sort(s, 2, 2 - sorted_on_scalar(s))
+                for gather in (gather_seconds, gather_firsts):
+                    gather(s, range(0, 2))
+                    gather(s, range(2, RG))
             elif n < RG:
-                sort(s, n, RG - n - sorted_on_scalar(s))
+                gather_firsts(s, exchanged(s))
 
         def band_sum(r, c, u):
             if 0 not in sbank:
@@ -217,10 +251,9 @@ def tile_relationalgraphconvolution_pa_kernel(
                 grp[s] = three.tile([P, RG * N], BF16, name="grp", align_bytes=64)
             bank = ring.tile([P, 512], F32, name="bank")
             for c in range(2):
-                src, first, apart = perm[s, a, c]
                 for u in range(2):
                     k0 = (c * 2 + u) * P
-                    w0 = first + u * apart
+                    src, w0 = perm[s, a, c][u]
                     nc.tensor.transpose(bank[:, k0 : k0 + P], src[:].bitcast(F32)[:, w0 : w0 + P], ident[:])
             if 0 <= RG * s + a - BAND_LAG < BAND_TILES:
                 for k in range(4):
@@ -249,12 +282,13 @@ def tile_relationalgraphconvolution_pa_kernel(
             for a in range(a0, a0 + n):
                 for c in range(2):
                     cols = slice(a * 256 + c * P, a * 256 + (c + 1) * P)
+                    f0 = (c + 2 * (a in exchanged(s))) * DE
                     nc.tensor.matmul_mx(
                         out=mx[s, a0][:, (a - a0) * DE : (a - a0 + 1) * DE],
                         lhsT=codes[s][:, cols].bitcast(FP8X4),
                         lhsT_scale=scales[s][:, cols],
-                        rhs=nf_codes[:, c * DE : (c + 1) * DE].bitcast(FP8X4),
-                        rhs_scale=nf_scales[:, c * DE : (c + 1) * DE],
+                        rhs=nf_codes[:, f0 : f0 + DE].bitcast(FP8X4),
+                        rhs_scale=nf_scales[:, f0 : f0 + DE],
                         start=(c == 0),
                         stop=(c == 1),
                     )
@@ -445,18 +479,24 @@ def tile_relationalgraphconvolution_pa_kernel(
                 load_rows(rel_rows, relation_features[0])
                 load_rows(scale_rows, Wb_scale.rearrange("o (r f) -> (o r) f", f=F))
             if s == 2:
-                nc.vector.quantize_mx(out=nf_codes[:].bitcast(FP8X4), scales=nf_scales[:], in_=nf_grp[:])
+                quantise_features(0)
+            if CATCH_UP < s < STEPS - 2 and exchanged(s + 2):
+                gather_seconds(s + 2, exchanged(s + 2))
             if s >= 1:
                 quantise(s - 1)
+            if s == REGROUP + 1:
+                quantise_features(1)
             if s == ROWS_PICK:
                 finish = [pick_own(relf, rel_rows, DR), pick_own(w_scale, scale_rows, F)]
             if it >= 0 and phase == 3:
                 collect_sums(it)
             if 1 <= s <= CATCH_UP:
                 sort_step(s + 1)
+            if s == CATCH_UP:
+                gather_seconds(s + 2, exchanged(s + 2))
             if s == 1:
                 nc.vector.tensor_copy(
-                    out=nf_grp[:].rearrange("p (c d t) -> p c d t", c=2, t=4),
+                    out=nf_grp[:, 0:1024].rearrange("p (c d t) -> p c d t", c=2, t=4),
                     in_=nf_raw[:].rearrange("p c (t d) -> p c d t", t=4),
                 )
             if CATCH_UP <= s < STEPS - 2:
@@ -466,6 +506,8 @@ def tile_relationalgraphconvolution_pa_kernel(
                     reduce_picked()
             for a in range(RG):
                 empty(s, a, turn(s, a))
+            if s == REGROUP:
+                regroup_features()
             if it >= 0 and phase == 2:
                 turn_sums(it)
             if it >= 0 and phase >= 2:
@@ -494,8 +536,6 @@ def tile_relationalgraphconvolution_pa_kernel(
             if s in project_at:
                 project(project_at[s], all_passes)
                 store(project_at[s])
-            if s + 2 < STEPS and sorted_on_scalar(s + 2):
-                sort(s + 2, RG - 1, 1, nc.scalar.copy)
             if s >= 1 and s != 2:
                 row_sums(s - 1, (0, 1) if phase == 1 else (1,))
             if it >= 0 and phase == 0:

@@ -15,20 +15,20 @@ RG = 4
 GROUPS = R // RG
 STEPS = IT * GROUPS
 GROUP = 8
+RUN = 16
+LEAD = 128
+PITCH = LEAD + N
 PASSES = F // 32
 PREFETCH = 5
-W0 = 4
-W_TURN = 9
-FIRST_PROJECT = 22
-CATCH_UP = 7
-BAND_TILES = 4
+HALVED = 7
+W_FROM = 8
+V_UNTIL = 6
+V_FROM = 21
+BAND_STEPS = 2
 BAND_LAG = 3
-W_LOAD = 1
-HALVED = 8
-ROWS_LOAD = 0
-ROWS_PICK = 5
-REGROUP = 3
-PROJECT_LAG = 10
+CATCH_UP = 7
+FIRST_PROJECT = W_FROM + 12
+PROJECT_LAG = 9
 
 F32 = mybir.dt.float32
 BF16 = mybir.dt.bfloat16
@@ -44,15 +44,17 @@ FLOPS = 2 * (R * N * N * DE + N * R * F * NB)
 
 
 def summed_on_vector(s):
-    return RG if s == STEPS - 1 else int(s >= FIRST_PROJECT - 1)
+    if s == STEPS - 1:
+        return RG
+    return 2 if s < V_UNTIL or s >= V_FROM else 0
 
 
-def summed_by_band(s):
-    return min(max(BAND_TILES - RG * s, 0), RG)
+def crossed(s):
+    return RG - summed_on_vector(s)
 
 
-def not_narrow(s):
-    return summed_on_vector(s) + summed_by_band(s)
+def summed_narrow(s):
+    return crossed(s) if s >= BAND_STEPS else 0
 
 
 def tile_relationalgraphconvolution_pa_kernel(
@@ -62,11 +64,10 @@ def tile_relationalgraphconvolution_pa_kernel(
     with ExitStack() as ctx:
         keep = ctx.enter_context(tc.tile_pool(name="keep", bufs=1))
         rawp = ctx.enter_context(tc.tile_pool(name="rawp", bufs=PREFETCH + 3))
-        onep = ctx.enter_context(tc.tile_pool(name="onep", bufs=8))
+        onep = ctx.enter_context(tc.tile_pool(name="onep", bufs=6))
         two = ctx.enter_context(tc.tile_pool(name="two", bufs=2))
         three = ctx.enter_context(tc.tile_pool(name="three", bufs=3))
-        four = ctx.enter_context(tc.tile_pool(name="four", bufs=5))
-        many = ctx.enter_context(tc.tile_pool(name="many", bufs=5))
+        many = ctx.enter_context(tc.tile_pool(name="many", bufs=6))
         ring = ctx.enter_context(tc.psum_pool(name="ring", bufs=6))
         sump = ctx.enter_context(tc.psum_pool(name="sump", bufs=1))
         ctx.enter_context(tc.manual_schedule())
@@ -74,46 +75,47 @@ def tile_relationalgraphconvolution_pa_kernel(
         ident = keep.tile([P, P], F32, name="ident", align_bytes=64)
         make_identity(nc, ident[:])
         rs = keep.tile([P, STEPS * RG], F32, name="rs", align_bytes=64)
-        patterns = [tuple(not_narrow(GROUPS * it + g) for g in range(GROUPS)) for it in range(IT)]
+        patterns = [
+            tuple((summed_narrow(s), summed_on_vector(s)) for s in range(GROUPS * it, GROUPS * (it + 1)))
+            for it in range(IT)
+        ]
+        parts = {key: 3 if any(n for m, n in key) else 2 for key in patterns}
         rep = {}
         for key in patterns:
             if key not in rep:
-                parts = 2 if key == patterns[0] or not sum(key) else 3
-                rep[key] = keep.tile([P, parts * P], F32, name="rep%d%d%d%d" % key, align_bytes=64)
-                if sum(key):
+                rep[key] = keep.tile([P, parts[key] * P], F32, name="rep%d" % len(rep), align_bytes=64)
+                if any(m < RG for m, n in key):
                     nc.vector.memset(rep[key][:], 0.0)
         ones = keep.tile([P, GROUP], BF16, name="ones", align_bytes=64)
         nc.vector.memset(ones[:], 1.0)
         band = keep.tile([P, 2 * P - GROUP], BF16, name="band", align_bytes=64)
         nc.vector.memset(band[:], 0.0)
         nc.vector.memset(band[:, P - GROUP : P], 1.0)
-        one = keep.tile([P, 1], F32, name="one", align_bytes=64)
-        nc.vector.memset(one[:], 1.0)
         pick = keep.tile([P, GROUP], F32, name="pick", align_bytes=64)
         nc.vector.tensor_reduce(
             out=pick[:], in_=ident[:].rearrange("p (g x) -> p x g", x=GROUP), axis=AXIS_X, op=ADD
         )
-        regroup = keep.tile([P, P], BF16, name="regroup", align_bytes=64)
-        nc.vector.tensor_copy(
-            out=regroup[:].rearrange("p (j h x) -> p j h x", h=2, x=GROUP),
-            in_=ident[:].rearrange("p (h j x) -> p j h x", h=2, x=GROUP),
-        )
+        select = keep.tile([P, 4 * P], BF16, name="select", align_bytes=64)
+        nc.vector.memset(select[:], 0.0)
+        for par in range(2):
+            nc.vector.tensor_copy(
+                out=select[:].rearrange("p (c a j b x) -> p c a j b x", c=2, a=2, b=2, x=GROUP)[:, :, par, :, par, :],
+                in_=ident[:].rearrange("p (c j x) -> p c j x", c=2, x=GROUP),
+            )
         nf_raw = keep.tile([P, 2, 4 * DE], BF16, name="nf_raw", align_bytes=64)
         nf_grp = keep.tile([P, 4 * 4 * DE], BF16, name="nf_grp", align_bytes=64)
         nf_codes = keep.tile([P, 4 * DE], U32, name="nf_codes", align_bytes=64)
         nf_scales = keep.tile([P, 4 * DE], U8, name="nf_scales", align_bytes=64)
         rel_rows = keep.tile([P, DR], BF16, name="rel_rows", align_bytes=64)
+        masked = keep.tile([P, DR], F32, name="masked", align_bytes=64)
         relf = keep.tile([P, 2 * 4], F32, name="relf", align_bytes=64)
-        scale_rows = keep.tile([P, F], F32, name="scale_rows", align_bytes=64)
-        w_scale = keep.tile([P, PASSES * 4], F32, name="w_scale", align_bytes=64)
         w_bytes = [keep.tile([P, R * F], U8, name="w_bytes%d" % h, align_bytes=64) for h in range(2)]
-        w_val = [keep.tile([P, R * F], BF16, name="w_val%d" % h, align_bytes=64) for h in range(2)]
-        w_grp = keep.tile([P, PASSES * NB * 4], BF16, name="w_grp", align_bytes=64)
+        w_sorted = [keep.tile([P, R * F], BF16, name="w_sorted%d" % h, align_bytes=64) for h in range(2)]
         w_codes = keep.tile([P, PASSES * NB], U32, name="w_codes", align_bytes=64)
         w_scales = keep.tile([P, PASSES * NB], U8, name="w_scales", align_bytes=64)
 
         raw = {}
-        perm = {}
+        window = {}
         grp = {}
         codes = {}
         scales = {}
@@ -127,15 +129,21 @@ def tile_relationalgraphconvolution_pa_kernel(
         scodes = {}
         sscales = {}
         obank = {}
+        w_spread = {}
+        w_val = {}
+        w_grp = {}
+
+        def rows_of(s, a0, n, first):
+            return raw[s][:, first + a0 * PITCH : first + (a0 + n) * PITCH].rearrange("p (a q) -> p a q", q=PITCH)
 
         def load(s, pieces=1):
             it, g = s // GROUPS, s % GROUPS
-            raw[s] = rawp.tile([P, RG * N], BF16, name="raw", align_bytes=64)
+            raw[s] = rawp.tile([P, LEAD + RG * PITCH], BF16, name="raw", align_bytes=256)
             n = RG // pieces
-            for a in range(pieces):
-                r0 = g * RG + a * n
+            for a0 in range(0, RG, n):
+                r0 = g * RG + a0
                 nc.sync.dma_start(
-                    out=raw[s][:, a * n * N : (a + 1) * n * N].rearrange("p (r j) -> p r j", j=N),
+                    out=rows_of(s, a0, n, LEAD)[:, :, 0:N],
                     in_=adj[0, r0 : r0 + n, it * P : (it + 1) * P, :].rearrange("r i j -> i r j"),
                 )
 
@@ -145,14 +153,28 @@ def tile_relationalgraphconvolution_pa_kernel(
                 for u in range(2):
                     nc.sync.dma_start(out=nf_raw[:, c, u * 2 * DE : (u + 1) * 2 * DE], in_=runs[c, u])
 
-        def regroup_features():
-            for c in range(2):
-                bank = ring.tile([P, 512], F32, name="bank")
-                nc.tensor.matmul(bank[:], lhsT=regroup[:], rhs=nf_raw[:, c, :], start=True, stop=True)
-                nc.scalar.copy(
-                    out=nf_grp[:, 1024 + c * 512 : 1024 + (c + 1) * 512].rearrange("p (d t) -> p d t", t=4),
-                    in_=bank[:].rearrange("p (t d) -> p d t", t=4),
-                )
+        def cross_features(c):
+            bank = ring.tile([P, 512], F32, name="bank")
+            for u in range(2):
+                for par in range(2):
+                    half = u if par == 0 else 1 - u
+                    nc.tensor.matmul(
+                        bank[:, u * 256 : (u + 1) * 256],
+                        lhsT=select[:, (2 * c + par) * P : (2 * c + par + 1) * P],
+                        rhs=nf_raw[:, 1 - par, half * 256 : (half + 1) * 256],
+                        start=(par == 0),
+                        stop=(par == 1),
+                    )
+            nc.scalar.copy(
+                out=nf_grp[:, 1024 + c * 512 : 1024 + (c + 1) * 512].rearrange("p (d t) -> p d t", t=4),
+                in_=bank[:].rearrange("p (t d) -> p d t", t=4),
+            )
+
+        def interleave_features():
+            nc.vector.tensor_copy(
+                out=nf_grp[:, 0:1024].rearrange("p (c d t) -> p c d t", c=2, t=4),
+                in_=nf_raw[:].rearrange("p c (t d) -> p c d t", t=4),
+            )
 
         def quantise_features(v):
             cols = slice(v * 256, (v + 1) * 256)
@@ -162,89 +184,55 @@ def tile_relationalgraphconvolution_pa_kernel(
                 in_=nf_grp[:, v * 1024 : (v + 1) * 1024],
             )
 
-        def load_rows(dst, rows):
-            nc.sync.dma_start(out=dst[:], in_=rows.partition_broadcast(GROUP).rearrange("x r f -> r x f"))
-
-        def pick_own(dst, rows, width):
-            masked = two.tile([P, width], F32, name="masked", align_bytes=64)
+        def mask_relation_rows():
             nc.vector.tensor_tensor(
                 out=masked[:].rearrange("p (m x e) -> p m x e", x=GROUP, e=2),
-                in0=rows[:].rearrange("p (m x e) -> p m x e", x=GROUP, e=2),
-                in1=pick[:].unsqueeze(1).unsqueeze(3).to_broadcast([P, width // 16, GROUP, 2]),
+                in0=rel_rows[:].rearrange("p (m x e) -> p m x e", x=GROUP, e=2),
+                in1=pick[:].unsqueeze(1).unsqueeze(3).to_broadcast([P, DR // 16, GROUP, 2]),
                 op=MULT,
             )
-            return lambda: nc.vector.tensor_reduce(
-                out=dst[:].rearrange("p (m e) -> p m e", e=2),
+
+        def pick_relation_values():
+            nc.vector.tensor_reduce(
+                out=relf[:].rearrange("p (m e) -> p m e", e=2),
                 in_=masked[:].rearrange("p (m x e) -> p m e x", x=GROUP, e=2),
                 axis=AXIS_X,
                 op=ADD,
             )
 
-        def sort(s, a0, n):
-            dst = onep.tile([P, N], BF16, name="permone", align_bytes=64)
-            for a in range(n):
+        def cross(s, a0, n):
+            for a in range(a0, a0 + n):
                 for c in range(2):
-                    h, k = divmod(2 * a + c, n)
-                    perm[s, a0 + a, c] = [(dst, ((2 * h + u) * n + k) * P) for u in range(2)]
-            nc.vector.tensor_copy(
-                out=dst[:].rearrange("p (h u q f) -> p h u q f", h=2, u=2, f=16),
-                in_=raw[s][:, a0 * N : (a0 + n) * N].rearrange("p (h q u f) -> p h u q f", h=2, u=2, f=16),
-            )
-
-        def exchanged(s):
-            return range(summed_on_vector(s), RG) if s > 3 else range(0)
-
-        def gather_seconds(s, tiles):
-            dst = four.tile([P, len(tiles) * 512], BF16, name="seconds", align_bytes=64)
-            for a in tiles:
-                for c in range(2):
-                    perm[s, a, c] = ((raw[s], (4 * a + 2 * c) * P), (dst, (2 * (a - tiles[0]) + c) * P))
-            rows = raw[s][:, tiles[0] * N : (tiles[-1] + 1) * N].rearrange("p (m h j u f) -> p m h j u f", h=2, j=8, u=2, f=16)
-            nc.vector.tensor_copy(
-                out=dst[:].rearrange("p (m j h f) -> p m h j f", j=8, h=2, f=16), in_=rows[:, :, :, :, 1, :]
-            )
-
-        def gather_firsts(s, tiles):
-            rows = raw[s][:, tiles[0] * N : (tiles[-1] + 1) * N].rearrange("p (m h j u f) -> p m h j u f", h=2, j=8, u=2, f=16)
-            nc.vector.tensor_copy(out=rows[:, :, 0, :, 1, :], in_=rows[:, :, 1, :, 0, :])
+                    first = a * PITCH // 2 + c * P
+                    window[s, a, c] = ((raw[s], first + (LEAD + N // 2) // 2), (raw[s], first + (LEAD - RUN) // 2))
+            odd = rows_of(s, a0, n, LEAD)[:, :, 0:N].rearrange("p a (h j o f) -> p a j h o f", h=2, o=2, f=RUN)
+            free = rows_of(s, a0, n, LEAD - RUN)[:, :, 0 : N + 4 * RUN]
+            free = free.rearrange("p a (h j o f) -> p a j h o f", h=2, o=2, f=RUN)
+            nc.vector.tensor_copy(out=free[:, :, 0:16, :, 0, :], in_=odd[:, :, :, ::-1, 1, :])
 
         def sort_and_sum(s, a):
-            dst = onep.tile([P, N], BF16, name="permone", align_bytes=64)
+            dst = onep.tile([P, N], BF16, name="sorted", align_bytes=64)
             for c in range(2):
-                perm[s, a, c] = [(dst, (2 * u + c) * P) for u in range(2)]
-            sorted_words = dst[:].rearrange("p (u q f) -> p u q f", u=2, f=16)
-            row = raw[s][:, a * N : (a + 1) * N].rearrange("p (q u f) -> p u q f", u=2, f=16)
-            total = rs[:, s * RG + a : s * RG + a + 1]
+                window[s, a, c] = [(dst, (2 * u + c) * P) for u in range(2)]
             nc.vector.tensor_scalar(
-                out=sorted_words, in0=row, scalar1=1.0, scalar2=None, op0=MULT, op1=ADD, accum_out=total
+                out=dst[:].rearrange("p (u q f) -> p u q f", u=2, f=RUN),
+                in0=raw[s][:, LEAD + a * PITCH : LEAD + a * PITCH + N].rearrange("p (q u f) -> p u q f", u=2, f=RUN),
+                scalar1=1.0,
+                scalar2=None,
+                op0=MULT,
+                op1=ADD,
+                accum_out=rs[:, s * RG + a : s * RG + a + 1],
             )
 
-        def sort_step(s):
-            n = summed_on_vector(s)
-            for a in range(summed_on_vector(s)):
+        def arrange(s):
+            n = crossed(s)
+            if n == RG and s <= HALVED:
+                cross(s, 0, 2)
+                cross(s, 2, 2)
+            elif n:
+                cross(s, 0, n)
+            for a in range(n, RG):
                 sort_and_sum(s, a)
-            if s <= 3:
-                for a in range(n, RG):
-                    sort(s, a, 1)
-            elif s <= HALVED:
-                for gather in (gather_seconds, gather_firsts):
-                    gather(s, range(0, 2))
-                    gather(s, range(2, RG))
-            elif n < RG:
-                gather_firsts(s, exchanged(s))
-
-        def band_sum(r, c, u):
-            if 0 not in sbank:
-                sbank[0] = sump.tile([P, 512], F32, name="sbank")
-            c0 = r % RG * N + c * 512
-            words = grp[r // RG][:, c0 : c0 + 512].rearrange("p (i u e) -> p u i e", u=2, e=2)
-            nc.tensor.matmul(
-                sbank[0][:, 0 : 2 * P].rearrange("p (i e) -> p i e", e=2),
-                lhsT=band[:, P - GROUP * (r + 1) : 2 * P - GROUP * (r + 1)],
-                rhs=words[:, u],
-                start=(r == 0 and c == 0 and u == 0),
-                stop=False,
-            )
 
         def turn(s, a):
             if a == 0:
@@ -253,11 +241,8 @@ def tile_relationalgraphconvolution_pa_kernel(
             for c in range(2):
                 for u in range(2):
                     k0 = (c * 2 + u) * P
-                    src, w0 = perm[s, a, c][u]
+                    src, w0 = window[s, a, c][u]
                     nc.tensor.transpose(bank[:, k0 : k0 + P], src[:].bitcast(F32)[:, w0 : w0 + P], ident[:])
-            if 0 <= RG * s + a - BAND_LAG < BAND_TILES:
-                for k in range(4):
-                    band_sum(RG * s + a - BAND_LAG, k // 2, k % 2)
             return bank
 
         def empty(s, a, bank, copy=nc.scalar.copy):
@@ -282,7 +267,7 @@ def tile_relationalgraphconvolution_pa_kernel(
             for a in range(a0, a0 + n):
                 for c in range(2):
                     cols = slice(a * 256 + c * P, a * 256 + (c + 1) * P)
-                    f0 = (c + 2 * (a in exchanged(s))) * DE
+                    f0 = (c + 2 * (a < crossed(s))) * DE
                     nc.tensor.matmul_mx(
                         out=mx[s, a0][:, (a - a0) * DE : (a - a0 + 1) * DE],
                         lhsT=codes[s][:, cols].bitcast(FP8X4),
@@ -293,33 +278,36 @@ def tile_relationalgraphconvolution_pa_kernel(
                         stop=(c == 1),
                     )
 
-        def keep_supports(s, a0=0, n=RG, copy=nc.scalar.copy):
-            it, r0 = s // GROUPS, s % GROUPS * RG + a0
-            if r0 == 0:
-                supn[it] = two.tile([P, R * DE], BF16, name="supn", align_bytes=64)
-            copy(
-                out=supn[it][:].rearrange("p (m r f) -> p m r f", r=R, f=16)[:, :, r0 : r0 + n, :],
-                in_=mx[s, a0][:, 0 : n * DE].rearrange("p (a m f) -> p m a f", a=n, f=16),
+        def keep_supports(s, a0=0, n=RG):
+            if s % 2 == 0 and a0 == 0:
+                supn[s // 2] = three.tile([P, 1024], BF16, name="supn", align_bytes=64)
+            halves = supn[s // 2][:, s % 2 * 512 : (s % 2 + 1) * 512].rearrange("p (u m f) -> p u m f", u=2, f=RUN)
+            nc.scalar.copy(
+                out=halves[:, :, 4 * a0 : 4 * (a0 + n), :],
+                in_=mx[s, a0][:, 0 : n * DE].rearrange("p (m u f) -> p u m f", u=2, f=RUN),
             )
 
-        def turn_supports(it, q0, n=2, copy=nc.scalar.copy):
-            if q0 == 0:
-                sgn[it] = two.tile([P, 2048], BF16, name="sgn", align_bytes=64)
+        def turn_supports(s0, n=2, copy=nc.scalar.copy):
+            if s0 % 2 == 0:
+                sgn[s0 // 2] = two.tile([P, 1024], BF16, name="sgn", align_bytes=64)
             bank = ring.tile([P, 512], F32, name="bank")
             for k in range(2 * n):
-                w0 = (2 * q0 + k) * P
-                nc.tensor.transpose(bank[:, k * P : (k + 1) * P], supn[it][:].bitcast(F32)[:, w0 : w0 + P], ident[:])
+                w0 = (s0 % 2 * 2 + k) * P
+                nc.tensor.transpose(
+                    bank[:, k * P : (k + 1) * P], supn[s0 // 2][:].bitcast(F32)[:, w0 : w0 + P], ident[:]
+                )
+            q0 = s0 % 2
             copy(
-                out=sgn[it][:, q0 * 512 : (q0 + n) * 512].bitcast(F32).rearrange("p (b i u) -> p b i u", b=n, u=2),
+                out=sgn[s0 // 2][:, q0 * 512 : (q0 + n) * 512].bitcast(F32).rearrange("p (b i u) -> p b i u", b=n, u=2),
                 in_=bank[:, 0 : n * 256].rearrange("p (b u i) -> p b i u", b=n, u=2),
             )
 
         def row_sums(s, halves=(0, 1)):
             it, g = s // GROUPS, s % GROUPS
-            if it not in wbank and not_narrow(s) < RG:
+            if it not in wbank and summed_narrow(s):
                 wbank[it] = sump.tile([P, 512], F32, name="wbank")
             for v in halves:
-                for a in range(not_narrow(s), RG):
+                for a in range(summed_narrow(s)):
                     k0 = v * P + (g * RG + a) * GROUP
                     for j in range(4):
                         c0 = a * N + j // 2 * 512 + v * 256
@@ -331,6 +319,21 @@ def tile_relationalgraphconvolution_pa_kernel(
                             stop=(j == 3),
                         )
 
+        def band_sum(s, a):
+            it, r = s // GROUPS, s % GROUPS * RG + a
+            if s == 0 and a == 0:
+                sbank[0] = sump.tile([P, 512], F32, name="sbank")
+            for c in range(2):
+                words = grp[s][:, a * N + c * 512 : a * N + (c + 1) * 512].rearrange("p (i u e) -> p u i e", u=2, e=2)
+                for u in range(2):
+                    nc.tensor.matmul(
+                        sbank[it][:, 0 : 2 * P].rearrange("p (i e) -> p i e", e=2),
+                        lhsT=band[:, P - GROUP * (r + 1) : 2 * P - GROUP * (r + 1)],
+                        rhs=words[:, u],
+                        start=(s == 0 and a == 0 and c == 0 and u == 0),
+                        stop=False,
+                    )
+
         def runs_of(it):
             key = patterns[it]
             starts = [g for g in range(GROUPS) if g == 0 or key[g] != key[g - 1]]
@@ -339,31 +342,31 @@ def tile_relationalgraphconvolution_pa_kernel(
         def keep_sums(it):
             dst = rep[patterns[it]][:, 0 : 2 * P].rearrange("p (v g m) -> p v g m", v=2, g=GROUPS)
             src = wbank[it][:, 0 : 2 * P].rearrange("p (v g m) -> p v g m", v=2, g=GROUPS)
-            for g0, g1, n in runs_of(it):
-                if n < RG:
-                    nc.scalar.copy(out=dst[:, :, g0:g1, n * GROUP :], in_=src[:, :, g0:g1, n * GROUP :])
+            for g0, g1, (m, n) in runs_of(it):
+                if m:
+                    nc.scalar.copy(out=dst[:, :, g0:g1, 0 : m * GROUP], in_=src[:, :, g0:g1, 0 : m * GROUP])
 
         def spread_sums(it):
-            dst = rep[patterns[it]][:, 2 * P : 3 * P].rearrange("p (g a x) -> p g a x", g=GROUPS, x=GROUP)
-            src = rs[:, it * R : (it + 1) * R].rearrange("p (g a) -> p g a", a=RG)
-            for g0, g1, n in runs_of(it):
+            for g0, g1, (m, n) in runs_of(it):
                 if n:
+                    dst = rep[patterns[it]][:, 2 * P : 3 * P].rearrange("p (g a x) -> p g a x", g=GROUPS, x=GROUP)
+                    src = rs[:, it * R : (it + 1) * R].rearrange("p (g a) -> p g a", a=RG)
                     nc.scalar.copy(
-                        out=dst[:, g0:g1, 0:n, :],
-                        in_=src[:, g0:g1, 0:n].unsqueeze(3).to_broadcast([P, g1 - g0, n, GROUP]),
+                        out=dst[:, g0:g1, RG - n :, :],
+                        in_=src[:, g0:g1, RG - n :].unsqueeze(3).to_broadcast([P, g1 - g0, n, GROUP]),
                     )
 
         def turn_sums(it):
             if it > 0:
                 sbank[it] = sump.tile([P, 512], F32, name="sbank")
-            parts = 3 if it > 0 and sum(patterns[it]) else 2
-            for v in range(parts):
+            last = parts[patterns[it]] - 1
+            for v in range(last + 1):
                 nc.tensor.matmul(
                     sbank[it][:, v * P : (v + 1) * P] if v < 2 else sbank[it][:, 0 : 2 * P : 2],
                     lhsT=rep[patterns[it]][:, v * P : (v + 1) * P],
                     rhs=ident[:],
                     start=(v == 0 and it > 0),
-                    stop=(v == parts - 1),
+                    stop=(v == last),
                     is_transpose=True,
                 )
 
@@ -373,10 +376,10 @@ def tile_relationalgraphconvolution_pa_kernel(
                 out=sums[it][:], in_=sbank[it][:, 0 : 2 * P].rearrange("p (i u) -> p i u", u=2), axis=AXIS_X, op=ADD
             )
 
-        def relation_part(it, b, engine):
+        def relation_part(it, b):
             if b == 0:
                 sgr[it] = two.tile([P, 1024], BF16, name="sgr", align_bytes=64)
-            engine.tensor_tensor(
+            nc.vector.tensor_tensor(
                 out=sgr[it][:, b * 512 : (b + 1) * 512].rearrange("p (i t) -> p i t", t=4),
                 in0=sums[it][:].unsqueeze(2).to_broadcast([P, P, 4]),
                 in1=relf[:, b * 4 : (b + 1) * 4].unsqueeze(1).to_broadcast([P, P, 4]),
@@ -391,12 +394,12 @@ def tile_relationalgraphconvolution_pa_kernel(
             nc.vector.quantize_mx(
                 out=scodes[it][:, cols].bitcast(FP8X4),
                 scales=sscales[it][:, cols],
-                in_=sgr[it][:] if q0 == 4 else sgn[it][:, q0 * 512 : (q0 + n) * 512],
+                in_=sgr[it][:] if q0 == 4 else sgn[2 * it + q0 // 2][:, q0 % 2 * 512 : (q0 % 2 + n) * 512],
             )
 
-        def project(it, passes):
+        def project(it, passes, first, last):
             for q in passes:
-                if q == 4:
+                if q == first:
                     obank[it] = ring.tile([P, 512], F32, name="bank")
                 nc.tensor.matmul_mx(
                     out=obank[it][:, 0:NB],
@@ -404,23 +407,40 @@ def tile_relationalgraphconvolution_pa_kernel(
                     lhsT_scale=sscales[it][:, q * P : (q + 1) * P],
                     rhs=w_codes[:, q * NB : (q + 1) * NB].bitcast(FP8X4),
                     rhs_scale=w_scales[:, q * NB : (q + 1) * NB],
-                    start=(q == 4),
-                    stop=(q == 3),
+                    start=(q == first),
+                    stop=(q == last),
                 )
 
         def store(it):
-            res = two.tile([P, NB], F32, name="res", align_bytes=64)
+            res = three.tile([P, NB], F32, name="res", align_bytes=64)
             nc.scalar.copy(out=res[:], in_=obank[it][:, 0:NB])
             nc.sync.dma_start(out=out[0, it * P : (it + 1) * P, :], in_=res[:])
 
-        def widen_weights(h, half):
-            r0 = half * R // 2
-            nc.vector.tensor_scalar(
-                out=w_val[h][:].rearrange("p (m r f) -> p r m f", r=R, f=16)[:, r0 : r0 + R // 2],
-                in0=w_bytes[h][:, r0 * F : (r0 + R // 2) * F].bitcast(FP8),
-                scalar1=one[:],
-                scalar2=None,
-                op0=MULT,
+        def load_weight_scales(g):
+            w_spread[g] = three.tile([P, RG * F], F32, name="w_spread", align_bytes=64)
+            row = Wb_scale.rearrange("o k -> (o k)")[g * RG * F : (g + 1) * RG * F]
+            nc.sync.dma_start(out=w_spread[g][:], in_=row.partition_broadcast(P))
+
+        def scale_weights(g, h):
+            w_val[g, h] = two.tile([P, RG * F], BF16, name="w_val", align_bytes=64)
+            nc.vector.tensor_tensor(
+                out=w_val[g, h][:],
+                in0=w_bytes[h][:, g * RG * F : (g + 1) * RG * F].bitcast(FP8),
+                in1=w_spread[g][:],
+                op=MULT,
+            )
+
+        def sort_weights(g, h):
+            rows = w_val[g, h][:].rearrange("p (a f) -> p a f", f=F)
+            node = w_sorted[h][:, 0 : R * DE].rearrange("p (u r m f) -> p u r m f", u=2, r=R, f=RUN)
+            nc.vector.tensor_copy(
+                out=node[:, :, g * RG : (g + 1) * RG],
+                in_=rows[:, :, 0:DE].rearrange("p a (m u f) -> p u a m f", u=2, f=RUN),
+            )
+            rel = w_sorted[h][:, R * DE : R * F].rearrange("p (m r f) -> p m r f", r=R, f=RUN)
+            nc.vector.tensor_copy(
+                out=rel[:, :, g * RG : (g + 1) * RG],
+                in_=rows[:, :, DE:F].rearrange("p a (m f) -> p m a f", f=RUN),
             )
 
         def turn_weights(q):
@@ -428,160 +448,136 @@ def tile_relationalgraphconvolution_pa_kernel(
             for u in range(2):
                 for h in range(2):
                     k0 = (u * 2 + h) * P
-                    w0 = (q * 2 + u) * P
-                    nc.tensor.transpose(bank[:, k0 : k0 + P], w_val[h][:].bitcast(F32)[:, w0 : w0 + P], ident[:])
+                    w0 = (u * GROUPS + q) * P if q < GROUPS else (2 * q + u) * P
+                    nc.tensor.transpose(bank[:, k0 : k0 + P], w_sorted[h][:].bitcast(F32)[:, w0 : w0 + P], ident[:])
+            w_grp[q] = two.tile([P, 4 * NB], BF16, name="w_grp", align_bytes=64)
             nc.scalar.copy(
-                out=w_grp[:, q * 1024 : (q + 1) * 1024].bitcast(F32).rearrange("p (n u) -> p n u", u=2),
+                out=w_grp[q][:].bitcast(F32).rearrange("p (n u) -> p n u", u=2),
                 in_=bank[:].rearrange("p (u n) -> p n u", u=2),
             )
 
-        def scale_weights(q):
-            values = w_grp[:, q * 1024 : (q + 1) * 1024].rearrange("p (n t) -> p n t", t=4)
-            nc.vector.tensor_tensor(
-                out=values,
-                in0=values,
-                in1=w_scale[:, q * 4 : (q + 1) * 4].unsqueeze(1).to_broadcast([P, NB, 4]),
-                op=MULT,
-            )
-
-        def quantise_weights(pair):
-            cols = slice(pair * 512, (pair + 1) * 512)
-            nc.vector.quantize_mx(
-                out=w_codes[:, cols].bitcast(FP8X4),
-                scales=w_scales[:, cols],
-                in_=w_grp[:, pair * 2048 : (pair + 1) * 2048],
-            )
+        def quantise_weights(q):
+            cols = slice(q * NB, (q + 1) * NB)
+            nc.vector.quantize_mx(out=w_codes[:, cols].bitcast(FP8X4), scales=w_scales[:, cols], in_=w_grp[q][:])
 
         all_passes = (4, 5, 0, 1, 2, 3)
-        load(0, 4)
+        project_at = {max(GROUPS * it + PROJECT_LAG, 2 * it + FIRST_PROJECT): it for it in range(IT)}
+        w_turn_at = {W_FROM + 2 + min(2 * q, q + 3): q for q in range(PASSES)}
+
+        load(0, 2)
+        load_features()
         load(1, 2)
         load(2, 2)
-        load_features()
-        load(3, 2)
-        for s in range(4, PREFETCH):
-            load(s, 2 if s <= HALVED else 1)
+        nc.sync.dma_start(
+            out=rel_rows[:], in_=relation_features[0].partition_broadcast(GROUP).rearrange("x r f -> r x f")
+        )
+        for s in range(3, PREFETCH):
+            load(s, 2)
 
-        project_at = {max(4 * it + PROJECT_LAG, 3 * it // 2 + FIRST_PROJECT): it for it in range(IT)}
-
-        sort_step(0)
-        sort_step(1)
-        for s in range(STEPS - 2):
-            w = s - W0
-            it, phase = (s - 4) // GROUPS, s % GROUPS
-            pair, stage = divmod(s - W_TURN, GROUPS)
-            weights = 0 <= pair < PASSES // 2
-            h = s - W_LOAD
-            if h in (0, 1):
-                nc.sync.dma_start(out=w_bytes[h][:], in_=Wb_bytes[h * P : (h + 1) * P, :])
+        arrange(0)
+        for s in range(STEPS - 1):
+            it, phase = s // GROUPS - 1, s % GROUPS
+            g, h = divmod(s - W_FROM, 2)
+            if s in (W_FROM - 5, W_FROM - 4):
+                k = s - (W_FROM - 5)
+                nc.sync.dma_start(out=w_bytes[k][:], in_=Wb_bytes[k * P : (k + 1) * P, :])
+            if 0 <= g + 2 < GROUPS and h == 1:
+                load_weight_scales(g + 2)
             if s + PREFETCH < STEPS:
                 load(s + PREFETCH, 2 if s + PREFETCH <= HALVED else 1)
-            if s == ROWS_LOAD:
-                load_rows(rel_rows, relation_features[0])
-                load_rows(scale_rows, Wb_scale.rearrange("o (r f) -> (o r) f", f=F))
-            if s == 2:
-                quantise_features(0)
-            if CATCH_UP < s < STEPS - 2 and exchanged(s + 2):
-                gather_seconds(s + 2, exchanged(s + 2))
+
+            if 0 <= g < GROUPS:
+                scale_weights(g, h)
             if s >= 1:
                 quantise(s - 1)
-            if s == REGROUP + 1:
-                quantise_features(1)
-            if s == ROWS_PICK:
-                finish = [pick_own(relf, rel_rows, DR), pick_own(w_scale, scale_rows, F)]
-            if it >= 0 and phase == 3:
-                collect_sums(it)
-            if 1 <= s <= CATCH_UP:
-                sort_step(s + 1)
-            if s == CATCH_UP:
-                gather_seconds(s + 2, exchanged(s + 2))
+            if s == 0:
+                interleave_features()
+            if s <= CATCH_UP:
+                arrange(s + 1)
             if s == 1:
-                nc.vector.tensor_copy(
-                    out=nf_grp[:, 0:1024].rearrange("p (c d t) -> p c d t", c=2, t=4),
-                    in_=nf_raw[:].rearrange("p c (t d) -> p c d t", t=4),
-                )
+                quantise_features(0)
+                quantise_features(1)
+            if s == 2:
+                mask_relation_rows()
+            if s == 3:
+                pick_relation_values()
+            if 0 <= g < GROUPS:
+                sort_weights(g, h)
+            if it >= 0 and phase == 2:
+                collect_sums(it)
             if CATCH_UP <= s < STEPS - 2:
-                sort_step(s + 2)
-            if s == ROWS_PICK:
-                for reduce_picked in finish:
-                    reduce_picked()
+                arrange(s + 2)
+            if s - 1 in w_turn_at:
+                quantise_weights(w_turn_at[s - 1])
+            if it >= 0 and phase == 1:
+                quantise_supports(it, 0)
+            if it >= 0 and phase == 2:
+                relation_part(it, 0)
+            if it >= 0 and phase == 3:
+                relation_part(it, 1)
+                quantise_supports(it, 2)
+            if it >= 1 and phase == 0:
+                quantise_supports(it - 1, 4)
+
+            if it >= 0 and phase == 1:
+                keep_sums(it)
+                spread_sums(it)
             for a in range(RG):
                 empty(s, a, turn(s, a))
-            if s == REGROUP:
-                regroup_features()
-            if it >= 0 and phase == 2:
+                if s == 0 and a in (1, 2):
+                    cross_features(a - 1)
+                k = RG * s + a - BAND_LAG
+                if 0 <= k < BAND_STEPS * RG and k % RG < 2:
+                    band_sum(k // RG, k % RG)
+            if s >= 4 and s % 2 == 0:
+                turn_supports(s - 4)
+            if it >= 0 and phase == 1:
                 turn_sums(it)
-            if it >= 0 and phase >= 2:
-                turn_supports(it, 2 * (phase - 2))
-            if weights and stage < 2:
-                turn_weights(2 * pair + stage)
-            if weights and stage in (1, 2):
-                scale_weights(2 * pair + stage - 1)
-            if 0 <= w < 4:
-                widen_weights(w // 2, w % 2)
-            if weights and stage == 3:
-                quantise_weights(pair)
-            if it >= 0 and phase == 3:
-                relation_part(it, 0, nc.vector)
-                quantise_supports(it, 0)
-            if it >= 1 and phase == 0:
-                relation_part(it - 1, 1, nc.vector)
-                quantise_supports(it - 1, 2)
-            if it >= 1 and phase == 1:
-                quantise_supports(it - 1, 4)
-            if s >= 1 and phase != 1:
-                row_sums(s - 1, (0, 1) if s == 2 else (0,))
+            if s in w_turn_at:
+                turn_weights(w_turn_at[s])
+            if s >= 1:
+                row_sums(s - 1, (0,))
             if s >= 2:
                 aggregate(s - 2)
                 keep_supports(s - 2)
             if s in project_at:
-                project(project_at[s], all_passes)
+                project(project_at[s], all_passes, 4, 3)
                 store(project_at[s])
-            if s >= 1 and s != 2:
-                row_sums(s - 1, (0, 1) if phase == 1 else (1,))
-            if it >= 0 and phase == 0:
-                keep_sums(it)
-            if it >= 1 and phase == 0 and sum(patterns[it]):
-                spread_sums(it)
+            if s >= 1:
+                row_sums(s - 1, (1,))
 
         s, it = STEPS - 1, IT - 1
-        quantise(s - 2)
-        for a in range(RG):
-            empty(s - 1, a, turn(s - 1, a))
-        turn_sums(it - 1)
-        collect_sums(it - 1)
-        for a in range(RG):
-            empty(s, a, turn(s, a), nc.scalar.copy if a % 2 else nc.vector.tensor_copy)
         quantise(s - 1)
-        quantise(s)
-        for j in range(2):
-            turn_supports(it - 1, 2 * j)
-            relation_part(it - 1, j, nc.vector)
-        row_sums(s - 2)
-        for k in (s - 3, s - 2):
-            aggregate(k)
-            keep_supports(k)
+        relation_part(it - 1, 1)
+        quantise_supports(it - 1, 2)
+        for a in range(RG):
+            empty(s, a, turn(s, a), nc.vector.tensor_copy if a % 2 else nc.scalar.copy)
         row_sums(s - 1)
+        aggregate(s - 2)
+        keep_supports(s - 2)
         keep_sums(it)
         spread_sums(it)
-        for k in (s - 1, s):
-            aggregate(k)
-            keep_supports(k)
-        quantise_supports(it - 1, 0)
-        quantise_supports(it - 1, 4)
-        quantise_supports(it - 1, 2)
+        aggregate(s - 1)
+        keep_supports(s - 1)
         turn_sums(it)
-        project(it - 2, all_passes)
+        quantise(s, 0, 2)
+        quantise_supports(it - 1, 4)
+        quantise(s, 2, 2)
         collect_sums(it)
-        relation_part(it, 0, nc.vector)
-        relation_part(it, 1, nc.vector)
-        store(it - 2)
-        for q in range(4):
-            turn_supports(it, q, 1)
-        project(it - 1, all_passes)
-        quantise_supports(it, 0, 1)
-        quantise_supports(it, 4)
-        for q in range(1, 4):
-            quantise_supports(it, q, 1)
+        aggregate(s, 0, 2)
+        turn_supports(s - 3)
+        aggregate(s, 2, 2)
+        for a0 in (0, 2):
+            keep_supports(s, a0, 2)
+        relation_part(it, 0)
+        quantise_supports(it, 0)
+        relation_part(it, 1)
+        turn_supports(s - 1, 1)
+        project(it - 1, all_passes, 4, 3)
+        turn_supports(s, 1)
         store(it - 1)
-        project(it, all_passes)
+        quantise_supports(it, 2, 1)
+        quantise_supports(it, 4)
+        quantise_supports(it, 3, 1)
+        project(it, (0, 1, 2, 4, 5, 3), 0, 3)
         store(it)

@@ -21,13 +21,14 @@ PITCH = LEAD + N
 PASSES = F // 32
 PREFETCH = 5
 HALVED = 7
-W_FROM = 8
+W_FROM = 7
+ROWS_AT = 4
 V_UNTIL = 6
-V_FROM = 21
+V_FROM = 22
 BAND_STEPS = 2
 BAND_LAG = 3
 CATCH_UP = 7
-FIRST_PROJECT = W_FROM + 12
+FIRST_PROJECT = W_FROM + 13
 PROJECT_LAG = 9
 
 F32 = mybir.dt.float32
@@ -107,10 +108,15 @@ def tile_relationalgraphconvolution_pa_kernel(
         nf_codes = keep.tile([P, 4 * DE], U32, name="nf_codes", align_bytes=64)
         nf_scales = keep.tile([P, 4 * DE], U8, name="nf_scales", align_bytes=64)
         rel_rows = keep.tile([P, DR], BF16, name="rel_rows", align_bytes=64)
-        masked = keep.tile([P, DR], F32, name="masked", align_bytes=64)
+        rel_masked = keep.tile([P, DR], F32, name="rel_masked", align_bytes=64)
+        scale_rows = keep.tile([P, F], F32, name="scale_rows", align_bytes=64)
+        scale_masked = keep.tile([P, F], F32, name="scale_masked", align_bytes=64)
+        w_scale = keep.tile([P, PASSES * 4], F32, name="w_scale", align_bytes=64)
+        one = keep.tile([P, 1], F32, name="one", align_bytes=64)
+        nc.vector.memset(one[:], 1.0)
         relf = keep.tile([P, 2 * 4], F32, name="relf", align_bytes=64)
         w_bytes = [keep.tile([P, R * F], U8, name="w_bytes%d" % h, align_bytes=64) for h in range(2)]
-        w_sorted = [keep.tile([P, R * F], BF16, name="w_sorted%d" % h, align_bytes=64) for h in range(2)]
+        w_val = [keep.tile([P, R * F], BF16, name="w_val%d" % h, align_bytes=64) for h in range(2)]
         w_codes = keep.tile([P, PASSES * NB], U32, name="w_codes", align_bytes=64)
         w_scales = keep.tile([P, PASSES * NB], U8, name="w_scales", align_bytes=64)
 
@@ -129,8 +135,6 @@ def tile_relationalgraphconvolution_pa_kernel(
         scodes = {}
         sscales = {}
         obank = {}
-        w_spread = {}
-        w_val = {}
         w_grp = {}
 
         def rows_of(s, a0, n, first):
@@ -184,17 +188,20 @@ def tile_relationalgraphconvolution_pa_kernel(
                 in_=nf_grp[:, v * 1024 : (v + 1) * 1024],
             )
 
-        def mask_relation_rows():
+        def load_rows(dst, rows):
+            nc.sync.dma_start(out=dst[:], in_=rows.partition_broadcast(GROUP).rearrange("x r f -> r x f"))
+
+        def mask_rows(masked, rows, width):
             nc.vector.tensor_tensor(
                 out=masked[:].rearrange("p (m x e) -> p m x e", x=GROUP, e=2),
-                in0=rel_rows[:].rearrange("p (m x e) -> p m x e", x=GROUP, e=2),
-                in1=pick[:].unsqueeze(1).unsqueeze(3).to_broadcast([P, DR // 16, GROUP, 2]),
+                in0=rows[:].rearrange("p (m x e) -> p m x e", x=GROUP, e=2),
+                in1=pick[:].unsqueeze(1).unsqueeze(3).to_broadcast([P, width // RUN, GROUP, 2]),
                 op=MULT,
             )
 
-        def pick_relation_values():
+        def pick_values(dst, masked):
             nc.vector.tensor_reduce(
-                out=relf[:].rearrange("p (m e) -> p m e", e=2),
+                out=dst[:].rearrange("p (m e) -> p m e", e=2),
                 in_=masked[:].rearrange("p (m x e) -> p m e x", x=GROUP, e=2),
                 axis=AXIS_X,
                 op=ADD,
@@ -279,26 +286,23 @@ def tile_relationalgraphconvolution_pa_kernel(
                     )
 
         def keep_supports(s, a0=0, n=RG):
-            if s % 2 == 0 and a0 == 0:
-                supn[s // 2] = three.tile([P, 1024], BF16, name="supn", align_bytes=64)
-            halves = supn[s // 2][:, s % 2 * 512 : (s % 2 + 1) * 512].rearrange("p (u m f) -> p u m f", u=2, f=RUN)
+            it, r0 = s // GROUPS, s % GROUPS * RG + a0
+            if r0 == 0:
+                supn[it] = two.tile([P, R * DE], BF16, name="supn", align_bytes=64)
             nc.scalar.copy(
-                out=halves[:, :, 4 * a0 : 4 * (a0 + n), :],
-                in_=mx[s, a0][:, 0 : n * DE].rearrange("p (m u f) -> p u m f", u=2, f=RUN),
+                out=supn[it][:].rearrange("p (m r f) -> p m r f", r=R, f=RUN)[:, :, r0 : r0 + n, :],
+                in_=mx[s, a0][:, 0 : n * DE].rearrange("p (a m f) -> p m a f", a=n, f=RUN),
             )
 
-        def turn_supports(s0, n=2, copy=nc.scalar.copy):
-            if s0 % 2 == 0:
-                sgn[s0 // 2] = two.tile([P, 1024], BF16, name="sgn", align_bytes=64)
+        def turn_supports(it, q0, n=2, copy=nc.scalar.copy):
+            if q0 == 0:
+                sgn[it] = two.tile([P, 2048], BF16, name="sgn", align_bytes=64)
             bank = ring.tile([P, 512], F32, name="bank")
             for k in range(2 * n):
-                w0 = (s0 % 2 * 2 + k) * P
-                nc.tensor.transpose(
-                    bank[:, k * P : (k + 1) * P], supn[s0 // 2][:].bitcast(F32)[:, w0 : w0 + P], ident[:]
-                )
-            q0 = s0 % 2
+                w0 = (2 * q0 + k) * P
+                nc.tensor.transpose(bank[:, k * P : (k + 1) * P], supn[it][:].bitcast(F32)[:, w0 : w0 + P], ident[:])
             copy(
-                out=sgn[s0 // 2][:, q0 * 512 : (q0 + n) * 512].bitcast(F32).rearrange("p (b i u) -> p b i u", b=n, u=2),
+                out=sgn[it][:, q0 * 512 : (q0 + n) * 512].bitcast(F32).rearrange("p (b i u) -> p b i u", b=n, u=2),
                 in_=bank[:, 0 : n * 256].rearrange("p (b u i) -> p b i u", b=n, u=2),
             )
 
@@ -394,7 +398,7 @@ def tile_relationalgraphconvolution_pa_kernel(
             nc.vector.quantize_mx(
                 out=scodes[it][:, cols].bitcast(FP8X4),
                 scales=sscales[it][:, cols],
-                in_=sgr[it][:] if q0 == 4 else sgn[2 * it + q0 // 2][:, q0 % 2 * 512 : (q0 % 2 + n) * 512],
+                in_=sgr[it][:] if q0 == 4 else sgn[it][:, q0 * 512 : (q0 + n) * 512],
             )
 
         def project(it, passes, first, last):
@@ -416,31 +420,14 @@ def tile_relationalgraphconvolution_pa_kernel(
             nc.scalar.copy(out=res[:], in_=obank[it][:, 0:NB])
             nc.sync.dma_start(out=out[0, it * P : (it + 1) * P, :], in_=res[:])
 
-        def load_weight_scales(g):
-            w_spread[g] = three.tile([P, RG * F], F32, name="w_spread", align_bytes=64)
-            row = Wb_scale.rearrange("o k -> (o k)")[g * RG * F : (g + 1) * RG * F]
-            nc.sync.dma_start(out=w_spread[g][:], in_=row.partition_broadcast(P))
-
-        def scale_weights(g, h):
-            w_val[g, h] = two.tile([P, RG * F], BF16, name="w_val", align_bytes=64)
-            nc.vector.tensor_tensor(
-                out=w_val[g, h][:],
-                in0=w_bytes[h][:, g * RG * F : (g + 1) * RG * F].bitcast(FP8),
-                in1=w_spread[g][:],
-                op=MULT,
-            )
-
-        def sort_weights(g, h):
-            rows = w_val[g, h][:].rearrange("p (a f) -> p a f", f=F)
-            node = w_sorted[h][:, 0 : R * DE].rearrange("p (u r m f) -> p u r m f", u=2, r=R, f=RUN)
-            nc.vector.tensor_copy(
-                out=node[:, :, g * RG : (g + 1) * RG],
-                in_=rows[:, :, 0:DE].rearrange("p a (m u f) -> p u a m f", u=2, f=RUN),
-            )
-            rel = w_sorted[h][:, R * DE : R * F].rearrange("p (m r f) -> p m r f", r=R, f=RUN)
-            nc.vector.tensor_copy(
-                out=rel[:, :, g * RG : (g + 1) * RG],
-                in_=rows[:, :, DE:F].rearrange("p a (m f) -> p m a f", f=RUN),
+        def widen_weights(h, half):
+            r0 = half * R // 2
+            nc.vector.tensor_scalar(
+                out=w_val[h][:].rearrange("p (m r f) -> p r m f", r=R, f=RUN)[:, r0 : r0 + R // 2],
+                in0=w_bytes[h][:, r0 * F : (r0 + R // 2) * F].bitcast(FP8),
+                scalar1=one[:],
+                scalar2=None,
+                op0=MULT,
             )
 
         def turn_weights(q):
@@ -448,12 +435,21 @@ def tile_relationalgraphconvolution_pa_kernel(
             for u in range(2):
                 for h in range(2):
                     k0 = (u * 2 + h) * P
-                    w0 = (u * GROUPS + q) * P if q < GROUPS else (2 * q + u) * P
-                    nc.tensor.transpose(bank[:, k0 : k0 + P], w_sorted[h][:].bitcast(F32)[:, w0 : w0 + P], ident[:])
-            w_grp[q] = two.tile([P, 4 * NB], BF16, name="w_grp", align_bytes=64)
+                    w0 = (2 * q + u) * P
+                    nc.tensor.transpose(bank[:, k0 : k0 + P], w_val[h][:].bitcast(F32)[:, w0 : w0 + P], ident[:])
+            w_grp[q] = three.tile([P, 4 * NB], BF16, name="w_grp", align_bytes=64)
             nc.scalar.copy(
                 out=w_grp[q][:].bitcast(F32).rearrange("p (n u) -> p n u", u=2),
                 in_=bank[:].rearrange("p (u n) -> p n u", u=2),
+            )
+
+        def scale_weights(q):
+            values = w_grp[q][:].rearrange("p (n t) -> p n t", t=4)
+            nc.vector.tensor_tensor(
+                out=values,
+                in0=values,
+                in1=w_scale[:, q * 4 : (q + 1) * 4].unsqueeze(1).to_broadcast([P, NB, 4]),
+                op=MULT,
             )
 
         def quantise_weights(q):
@@ -462,32 +458,29 @@ def tile_relationalgraphconvolution_pa_kernel(
 
         all_passes = (4, 5, 0, 1, 2, 3)
         project_at = {max(GROUPS * it + PROJECT_LAG, 2 * it + FIRST_PROJECT): it for it in range(IT)}
-        w_turn_at = {W_FROM + 2 + min(2 * q, q + 3): q for q in range(PASSES)}
+        w_turn_at = {W_FROM + 4 + 4 * q // 3: q for q in range(PASSES)}
 
         load(0, 2)
         load_features()
         load(1, 2)
         load(2, 2)
-        nc.sync.dma_start(
-            out=rel_rows[:], in_=relation_features[0].partition_broadcast(GROUP).rearrange("x r f -> r x f")
-        )
         for s in range(3, PREFETCH):
             load(s, 2)
 
         arrange(0)
         for s in range(STEPS - 1):
             it, phase = s // GROUPS - 1, s % GROUPS
-            g, h = divmod(s - W_FROM, 2)
-            if s in (W_FROM - 5, W_FROM - 4):
-                k = s - (W_FROM - 5)
-                nc.sync.dma_start(out=w_bytes[k][:], in_=Wb_bytes[k * P : (k + 1) * P, :])
-            if 0 <= g + 2 < GROUPS and h == 1:
-                load_weight_scales(g + 2)
+            w = s - W_FROM
+            if w in (-5, -4):
+                nc.sync.dma_start(out=w_bytes[w + 5][:], in_=Wb_bytes[(w + 5) * P : (w + 6) * P, :])
+            if s == 0:
+                load_rows(rel_rows, relation_features[0])
+                load_rows(scale_rows, Wb_scale.rearrange("o (r f) -> (o r) f", f=F))
             if s + PREFETCH < STEPS:
                 load(s + PREFETCH, 2 if s + PREFETCH <= HALVED else 1)
 
-            if 0 <= g < GROUPS:
-                scale_weights(g, h)
+            if s - 1 in w_turn_at:
+                scale_weights(w_turn_at[s - 1])
             if s >= 1:
                 quantise(s - 1)
             if s == 0:
@@ -497,27 +490,28 @@ def tile_relationalgraphconvolution_pa_kernel(
             if s == 1:
                 quantise_features(0)
                 quantise_features(1)
-            if s == 2:
-                mask_relation_rows()
-            if s == 3:
-                pick_relation_values()
-            if 0 <= g < GROUPS:
-                sort_weights(g, h)
+            if s == ROWS_AT:
+                mask_rows(rel_masked, rel_rows, DR)
+                mask_rows(scale_masked, scale_rows, F)
+            if s == ROWS_AT + 1:
+                pick_values(relf, rel_masked)
+                pick_values(w_scale, scale_masked)
             if it >= 0 and phase == 2:
                 collect_sums(it)
             if CATCH_UP <= s < STEPS - 2:
                 arrange(s + 2)
-            if s - 1 in w_turn_at:
-                quantise_weights(w_turn_at[s - 1])
-            if it >= 0 and phase == 1:
-                quantise_supports(it, 0)
+            if 0 <= w < 4:
+                widen_weights(w // 2, w % 2)
+            if s - 2 in w_turn_at:
+                quantise_weights(w_turn_at[s - 2])
             if it >= 0 and phase == 2:
                 relation_part(it, 0)
             if it >= 0 and phase == 3:
                 relation_part(it, 1)
-                quantise_supports(it, 2)
+                quantise_supports(it, 0)
             if it >= 1 and phase == 0:
                 quantise_supports(it - 1, 4)
+                quantise_supports(it - 1, 2)
 
             if it >= 0 and phase == 1:
                 keep_sums(it)
@@ -529,8 +523,8 @@ def tile_relationalgraphconvolution_pa_kernel(
                 k = RG * s + a - BAND_LAG
                 if 0 <= k < BAND_STEPS * RG and k % RG < 2:
                     band_sum(k // RG, k % RG)
-            if s >= 4 and s % 2 == 0:
-                turn_supports(s - 4)
+            if it >= 0 and phase >= 2:
+                turn_supports(it, 2 * (phase - 2))
             if it >= 0 and phase == 1:
                 turn_sums(it)
             if s in w_turn_at:
@@ -549,9 +543,10 @@ def tile_relationalgraphconvolution_pa_kernel(
         s, it = STEPS - 1, IT - 1
         quantise(s - 1)
         relation_part(it - 1, 1)
-        quantise_supports(it - 1, 2)
+        quantise_supports(it - 1, 0)
         for a in range(RG):
             empty(s, a, turn(s, a), nc.vector.tensor_copy if a % 2 else nc.scalar.copy)
+        turn_supports(it - 1, 2)
         row_sums(s - 1)
         aggregate(s - 2)
         keep_supports(s - 2)
@@ -563,21 +558,19 @@ def tile_relationalgraphconvolution_pa_kernel(
         quantise(s, 0, 2)
         quantise_supports(it - 1, 4)
         quantise(s, 2, 2)
+        quantise_supports(it - 1, 2)
         collect_sums(it)
-        aggregate(s, 0, 2)
-        turn_supports(s - 3)
-        aggregate(s, 2, 2)
         for a0 in (0, 2):
+            aggregate(s, a0, 2)
             keep_supports(s, a0, 2)
         relation_part(it, 0)
-        quantise_supports(it, 0)
         relation_part(it, 1)
-        turn_supports(s - 1, 1)
         project(it - 1, all_passes, 4, 3)
-        turn_supports(s, 1)
-        store(it - 1)
-        quantise_supports(it, 2, 1)
+        for q in range(4):
+            turn_supports(it, q, 1)
         quantise_supports(it, 4)
-        quantise_supports(it, 3, 1)
-        project(it, (0, 1, 2, 4, 5, 3), 0, 3)
+        for q in range(4):
+            quantise_supports(it, q, 1)
+        store(it - 1)
+        project(it, all_passes, 4, 3)
         store(it)

@@ -21,14 +21,14 @@ PITCH = LEAD + N
 PASSES = F // 32
 PREFETCH = 5
 HALVED = 7
-W_FROM = 7
+W_FROM = 5
 ROWS_AT = 4
-V_UNTIL = 6
-V_FROM = 22
+V_UNTIL = 3
+V_FROM = 29
 BAND_STEPS = 2
 BAND_LAG = 3
-CATCH_UP = 7
-FIRST_PROJECT = W_FROM + 13
+CATCH_UP = 5
+FIRST_PROJECT = W_FROM + 18
 PROJECT_LAG = 9
 
 F32 = mybir.dt.float32
@@ -45,7 +45,7 @@ FLOPS = 2 * (R * N * N * DE + N * R * F * NB)
 
 
 def summed_on_vector(s):
-    if s == STEPS - 1:
+    if s == STEPS - 1 or (s >= 2 * GROUPS and s % GROUPS == 0):
         return RG
     return 2 if s < V_UNTIL or s >= V_FROM else 0
 
@@ -65,7 +65,7 @@ def tile_relationalgraphconvolution_pa_kernel(
     with ExitStack() as ctx:
         keep = ctx.enter_context(tc.tile_pool(name="keep", bufs=1))
         rawp = ctx.enter_context(tc.tile_pool(name="rawp", bufs=PREFETCH + 3))
-        onep = ctx.enter_context(tc.tile_pool(name="onep", bufs=6))
+        onep = ctx.enter_context(tc.tile_pool(name="onep", bufs=8))
         two = ctx.enter_context(tc.tile_pool(name="two", bufs=2))
         three = ctx.enter_context(tc.tile_pool(name="three", bufs=3))
         many = ctx.enter_context(tc.tile_pool(name="many", bufs=6))
@@ -85,17 +85,12 @@ def tile_relationalgraphconvolution_pa_kernel(
         for key in patterns:
             if key not in rep:
                 rep[key] = keep.tile([P, parts[key] * P], F32, name="rep%d" % len(rep), align_bytes=64)
-                if any(m < RG for m, n in key):
-                    nc.vector.memset(rep[key][:], 0.0)
         ones = keep.tile([P, GROUP], BF16, name="ones", align_bytes=64)
         nc.vector.memset(ones[:], 1.0)
         band = keep.tile([P, 2 * P - GROUP], BF16, name="band", align_bytes=64)
         nc.vector.memset(band[:], 0.0)
         nc.vector.memset(band[:, P - GROUP : P], 1.0)
         pick = keep.tile([P, GROUP], F32, name="pick", align_bytes=64)
-        nc.vector.tensor_reduce(
-            out=pick[:], in_=ident[:].rearrange("p (g x) -> p x g", x=GROUP), axis=AXIS_X, op=ADD
-        )
         select = keep.tile([P, 4 * P], BF16, name="select", align_bytes=64)
         nc.vector.memset(select[:], 0.0)
         for par in range(2):
@@ -215,7 +210,10 @@ def tile_relationalgraphconvolution_pa_kernel(
             odd = rows_of(s, a0, n, LEAD)[:, :, 0:N].rearrange("p a (h j o f) -> p a j h o f", h=2, o=2, f=RUN)
             free = rows_of(s, a0, n, LEAD - RUN)[:, :, 0 : N + 4 * RUN]
             free = free.rearrange("p a (h j o f) -> p a j h o f", h=2, o=2, f=RUN)
-            nc.vector.tensor_copy(out=free[:, :, 0:16, :, 0, :], in_=odd[:, :, :, ::-1, 1, :])
+            dst, src = free[:, :, 0:16, :, 0, :], odd[:, :, :, ::-1, 1, :]
+            if n == 1:
+                dst, src = [v[:, 0].rearrange("p j h (k f) -> p k j h f", k=2) for v in (dst, src)]
+            nc.vector.tensor_copy(out=dst, in_=src)
 
         def sort_and_sum(s, a):
             dst = onep.tile([P, N], BF16, name="sorted", align_bytes=64)
@@ -233,7 +231,10 @@ def tile_relationalgraphconvolution_pa_kernel(
 
         def arrange(s):
             n = crossed(s)
-            if n == RG and s <= HALVED:
+            if s == 0:
+                cross(s, 0, 1)
+                cross(s, 1, 1)
+            elif n == RG and s <= HALVED:
                 cross(s, 0, 2)
                 cross(s, 2, 2)
             elif n:
@@ -380,13 +381,12 @@ def tile_relationalgraphconvolution_pa_kernel(
                 out=sums[it][:], in_=sbank[it][:, 0 : 2 * P].rearrange("p (i u) -> p i u", u=2), axis=AXIS_X, op=ADD
             )
 
-        def relation_part(it, b):
-            if b == 0:
-                sgr[it] = two.tile([P, 1024], BF16, name="sgr", align_bytes=64)
-            nc.vector.tensor_tensor(
-                out=sgr[it][:, b * 512 : (b + 1) * 512].rearrange("p (i t) -> p i t", t=4),
-                in0=sums[it][:].unsqueeze(2).to_broadcast([P, P, 4]),
-                in1=relf[:, b * 4 : (b + 1) * 4].unsqueeze(1).to_broadcast([P, P, 4]),
+        def relation_part(it, engine):
+            sgr[it] = two.tile([P, 1024], BF16, name="sgr", align_bytes=64)
+            engine.tensor_tensor(
+                out=sgr[it][:].rearrange("p (b i t) -> p b i t", b=2, t=4),
+                in0=sums[it][:].unsqueeze(1).unsqueeze(3).to_broadcast([P, 2, P, 4]),
+                in1=relf[:].rearrange("p (b t) -> p b t", t=4).unsqueeze(2).to_broadcast([P, 2, P, 4]),
                 op=MULT,
             )
 
@@ -437,14 +437,15 @@ def tile_relationalgraphconvolution_pa_kernel(
                     k0 = (u * 2 + h) * P
                     w0 = (2 * q + u) * P
                     nc.tensor.transpose(bank[:, k0 : k0 + P], w_val[h][:].bitcast(F32)[:, w0 : w0 + P], ident[:])
-            w_grp[q] = three.tile([P, 4 * NB], BF16, name="w_grp", align_bytes=64)
+            if q % 2 == 0:
+                w_grp[q // 2] = two.tile([P, 8 * NB], BF16, name="w_grp", align_bytes=64)
             nc.scalar.copy(
-                out=w_grp[q][:].bitcast(F32).rearrange("p (n u) -> p n u", u=2),
+                out=w_grp[q // 2][:, q % 2 * 1024 : (q % 2 + 1) * 1024].bitcast(F32).rearrange("p (n u) -> p n u", u=2),
                 in_=bank[:].rearrange("p (u n) -> p n u", u=2),
             )
 
         def scale_weights(q):
-            values = w_grp[q][:].rearrange("p (n t) -> p n t", t=4)
+            values = w_grp[q // 2][:, q % 2 * 1024 : (q % 2 + 1) * 1024].rearrange("p (n t) -> p n t", t=4)
             nc.vector.tensor_tensor(
                 out=values,
                 in0=values,
@@ -452,15 +453,16 @@ def tile_relationalgraphconvolution_pa_kernel(
                 op=MULT,
             )
 
-        def quantise_weights(q):
-            cols = slice(q * NB, (q + 1) * NB)
-            nc.vector.quantize_mx(out=w_codes[:, cols].bitcast(FP8X4), scales=w_scales[:, cols], in_=w_grp[q][:])
+        def quantise_weights(pair):
+            cols = slice(pair * 2 * NB, (pair + 1) * 2 * NB)
+            nc.vector.quantize_mx(out=w_codes[:, cols].bitcast(FP8X4), scales=w_scales[:, cols], in_=w_grp[pair][:])
 
         all_passes = (4, 5, 0, 1, 2, 3)
-        project_at = {max(GROUPS * it + PROJECT_LAG, 2 * it + FIRST_PROJECT): it for it in range(IT)}
-        w_turn_at = {W_FROM + 4 + 4 * q // 3: q for q in range(PASSES)}
+        project_at = {max(GROUPS * it + PROJECT_LAG, it + FIRST_PROJECT): it for it in range(IT)}
+        w_turn_at = {W_FROM + 5 + 2 * q: q for q in range(PASSES)}
+        widen_at = [s for s in range(W_FROM, W_FROM + 5) if s % GROUPS != 2]
 
-        load(0, 2)
+        load(0, 4)
         load_features()
         load(1, 2)
         load(2, 2)
@@ -468,21 +470,25 @@ def tile_relationalgraphconvolution_pa_kernel(
             load(s, 2)
 
         arrange(0)
+        nc.vector.tensor_reduce(out=pick[:], in_=ident[:].rearrange("p (g x) -> p x g", x=GROUP), axis=AXIS_X, op=ADD)
+        to_clear = [key for key in rep if any(m < RG for m, n in key)]
         for s in range(STEPS - 1):
             it, phase = s // GROUPS - 1, s % GROUPS
             w = s - W_FROM
-            if w in (-5, -4):
-                nc.sync.dma_start(out=w_bytes[w + 5][:], in_=Wb_bytes[(w + 5) * P : (w + 6) * P, :])
+            if w in (-4, -3):
+                nc.sync.dma_start(out=w_bytes[w + 4][:], in_=Wb_bytes[(w + 4) * P : (w + 5) * P, :])
             if s == 0:
                 load_rows(rel_rows, relation_features[0])
                 load_rows(scale_rows, Wb_scale.rearrange("o (r f) -> (o r) f", f=F))
             if s + PREFETCH < STEPS:
                 load(s + PREFETCH, 2 if s + PREFETCH <= HALVED else 1)
 
-            if s - 1 in w_turn_at:
-                scale_weights(w_turn_at[s - 1])
             if s >= 1:
                 quantise(s - 1)
+            if s - 1 in w_turn_at:
+                scale_weights(w_turn_at[s - 1])
+            if s < len(to_clear):
+                nc.vector.memset(rep[to_clear[s]][:], 0.0)
             if s == 0:
                 interleave_features()
             if s <= CATCH_UP:
@@ -496,22 +502,19 @@ def tile_relationalgraphconvolution_pa_kernel(
             if s == ROWS_AT + 1:
                 pick_values(relf, rel_masked)
                 pick_values(w_scale, scale_masked)
+            if s in widen_at:
+                widen_weights(*divmod(widen_at.index(s), 2))
             if it >= 0 and phase == 2:
                 collect_sums(it)
+                relation_part(it, nc.gpsimd if s + 2 < STEPS else nc.vector)
             if CATCH_UP <= s < STEPS - 2:
                 arrange(s + 2)
-            if 0 <= w < 4:
-                widen_weights(w // 2, w % 2)
-            if s - 2 in w_turn_at:
-                quantise_weights(w_turn_at[s - 2])
-            if it >= 0 and phase == 2:
-                relation_part(it, 0)
+            if w_turn_at.get(s - 1, 0) % 2:
+                quantise_weights(w_turn_at[s - 1] // 2)
             if it >= 0 and phase == 3:
-                relation_part(it, 1)
-                quantise_supports(it, 0)
+                quantise_supports(it, 4)
             if it >= 1 and phase == 0:
-                quantise_supports(it - 1, 4)
-                quantise_supports(it - 1, 2)
+                quantise_supports(it - 1, 0, 4)
 
             if it >= 0 and phase == 1:
                 keep_sums(it)
@@ -525,6 +528,8 @@ def tile_relationalgraphconvolution_pa_kernel(
                     band_sum(k // RG, k % RG)
             if it >= 0 and phase >= 2:
                 turn_supports(it, 2 * (phase - 2))
+            if s == STEPS - 2:
+                turn_supports(it, 2)
             if it >= 0 and phase == 1:
                 turn_sums(it)
             if s in w_turn_at:
@@ -542,35 +547,32 @@ def tile_relationalgraphconvolution_pa_kernel(
 
         s, it = STEPS - 1, IT - 1
         quantise(s - 1)
-        relation_part(it - 1, 1)
-        quantise_supports(it - 1, 0)
+        quantise_supports(it - 1, 0, 4)
+        quantise_supports(it - 1, 4)
         for a in range(RG):
-            empty(s, a, turn(s, a), nc.vector.tensor_copy if a % 2 else nc.scalar.copy)
-        turn_supports(it - 1, 2)
+            empty(s, a, turn(s, a), nc.vector.tensor_copy if a == 3 else nc.scalar.copy)
         row_sums(s - 1)
-        aggregate(s - 2)
-        keep_supports(s - 2)
         keep_sums(it)
         spread_sums(it)
+        aggregate(s - 2)
+        keep_supports(s - 2)
         aggregate(s - 1)
         keep_supports(s - 1)
         turn_sums(it)
         quantise(s, 0, 2)
-        quantise_supports(it - 1, 4)
         quantise(s, 2, 2)
-        quantise_supports(it - 1, 2)
         collect_sums(it)
         for a0 in (0, 2):
             aggregate(s, a0, 2)
             keep_supports(s, a0, 2)
-        relation_part(it, 0)
-        relation_part(it, 1)
+        relation_part(it, nc.vector)
         project(it - 1, all_passes, 4, 3)
         for q in range(4):
             turn_supports(it, q, 1)
-        quantise_supports(it, 4)
-        for q in range(4):
-            quantise_supports(it, q, 1)
         store(it - 1)
-        project(it, all_passes, 4, 3)
+        quantise_supports(it, 0, 1)
+        quantise_supports(it, 4)
+        for q in range(1, 4):
+            quantise_supports(it, q, 1)
+        project(it, (0, 4, 5, 1, 2, 3), 0, 3)
         store(it)

@@ -16,6 +16,7 @@ GROUPS = R // RG
 STEPS = IT * GROUPS
 GROUP = 8
 RUN = 16
+BANKS = 8
 LEAD = 128
 PITCH = LEAD + N
 PASSES = F // 32
@@ -24,10 +25,10 @@ HALVED = 7
 W_FROM = 5
 ROWS_AT = 4
 V_UNTIL = 3
-V_FROM = 29
+V_FROM = 25
 BAND_STEPS = 2
 BAND_LAG = 3
-CATCH_UP = 5
+CATCH_UP = 7
 FIRST_PROJECT = W_FROM + 18
 PROJECT_LAG = 9
 
@@ -45,7 +46,7 @@ FLOPS = 2 * (R * N * N * DE + N * R * F * NB)
 
 
 def summed_on_vector(s):
-    if s == STEPS - 1 or (s >= 2 * GROUPS and s % GROUPS == 0):
+    if s in (2 * GROUPS - 1, STEPS - 1) or (s > 2 * GROUPS and s % GROUPS == 0):
         return RG
     return 2 if s < V_UNTIL or s >= V_FROM else 0
 
@@ -69,8 +70,7 @@ def tile_relationalgraphconvolution_pa_kernel(
         two = ctx.enter_context(tc.tile_pool(name="two", bufs=2))
         three = ctx.enter_context(tc.tile_pool(name="three", bufs=3))
         many = ctx.enter_context(tc.tile_pool(name="many", bufs=6))
-        ring = ctx.enter_context(tc.psum_pool(name="ring", bufs=6))
-        sump = ctx.enter_context(tc.psum_pool(name="sump", bufs=1))
+        psum = ctx.enter_context(tc.psum_pool(name="psum", bufs=1))
         ctx.enter_context(tc.manual_schedule())
 
         ident = keep.tile([P, P], F32, name="ident", align_bytes=64)
@@ -121,8 +121,6 @@ def tile_relationalgraphconvolution_pa_kernel(
         codes = {}
         scales = {}
         mx = {}
-        wbank = {}
-        sbank = {}
         sums = {}
         supn = {}
         sgn = {}
@@ -131,6 +129,22 @@ def tile_relationalgraphconvolution_pa_kernel(
         sscales = {}
         obank = {}
         w_grp = {}
+
+        free_banks = list(range(BANKS - 2))
+        held = {}
+
+        def take_bank():
+            k = free_banks.pop(0)
+            bank = psum.tile([P, 512], F32, name="bank%d" % k)
+            held[k] = bank
+            return bank
+
+        def give_bank(bank):
+            free_banks.append([k for k in held if held[k] is bank][0])
+
+        sums_bank = psum.tile([P, 512], F32, name="bank%d" % (BANKS - 1))
+        first_sums = psum.tile([P, 512], F32, name="bank%d" % (BANKS - 2))
+        held[BANKS - 2] = first_sums
 
         def rows_of(s, a0, n, first):
             return raw[s][:, first + a0 * PITCH : first + (a0 + n) * PITCH].rearrange("p (a q) -> p a q", q=PITCH)
@@ -153,7 +167,7 @@ def tile_relationalgraphconvolution_pa_kernel(
                     nc.sync.dma_start(out=nf_raw[:, c, u * 2 * DE : (u + 1) * 2 * DE], in_=runs[c, u])
 
         def cross_features(c):
-            bank = ring.tile([P, 512], F32, name="bank")
+            bank = take_bank()
             for u in range(2):
                 for par in range(2):
                     half = u if par == 0 else 1 - u
@@ -168,6 +182,7 @@ def tile_relationalgraphconvolution_pa_kernel(
                 out=nf_grp[:, 1024 + c * 512 : 1024 + (c + 1) * 512].rearrange("p (d t) -> p d t", t=4),
                 in_=bank[:].rearrange("p (t d) -> p d t", t=4),
             )
+            give_bank(bank)
 
         def interleave_features():
             nc.vector.tensor_copy(
@@ -245,7 +260,7 @@ def tile_relationalgraphconvolution_pa_kernel(
         def turn(s, a):
             if a == 0:
                 grp[s] = three.tile([P, RG * N], BF16, name="grp", align_bytes=64)
-            bank = ring.tile([P, 512], F32, name="bank")
+            bank = take_bank()
             for c in range(2):
                 for u in range(2):
                     k0 = (c * 2 + u) * P
@@ -258,6 +273,7 @@ def tile_relationalgraphconvolution_pa_kernel(
                 out=grp[s][:, a * N : (a + 1) * N].bitcast(F32).rearrange("p (c i u) -> p c i u", c=2, u=2),
                 in_=bank[:].rearrange("p (c u i) -> p c i u", c=2, u=2),
             )
+            give_bank(bank)
 
         def quantise(s, a0=0, n=RG):
             if a0 == 0:
@@ -271,7 +287,7 @@ def tile_relationalgraphconvolution_pa_kernel(
             )
 
         def aggregate(s, a0=0, n=RG):
-            mx[s, a0] = ring.tile([P, 512], F32, name="bank")
+            mx[s, a0] = take_bank()
             for a in range(a0, a0 + n):
                 for c in range(2):
                     cols = slice(a * 256 + c * P, a * 256 + (c + 1) * P)
@@ -294,45 +310,50 @@ def tile_relationalgraphconvolution_pa_kernel(
                 out=supn[it][:].rearrange("p (m r f) -> p m r f", r=R, f=RUN)[:, :, r0 : r0 + n, :],
                 in_=mx[s, a0][:, 0 : n * DE].rearrange("p (a m f) -> p m a f", a=n, f=RUN),
             )
+            give_bank(mx[s, a0])
 
         def turn_supports(it, q0, n=2, copy=nc.scalar.copy):
             if q0 == 0:
                 sgn[it] = two.tile([P, 2048], BF16, name="sgn", align_bytes=64)
-            bank = ring.tile([P, 512], F32, name="bank")
+            bank = take_bank()
             for k in range(2 * n):
                 w0 = (2 * q0 + k) * P
                 nc.tensor.transpose(bank[:, k * P : (k + 1) * P], supn[it][:].bitcast(F32)[:, w0 : w0 + P], ident[:])
-            copy(
-                out=sgn[it][:, q0 * 512 : (q0 + n) * 512].bitcast(F32).rearrange("p (b i u) -> p b i u", b=n, u=2),
-                in_=bank[:, 0 : n * 256].rearrange("p (b u i) -> p b i u", b=n, u=2),
-            )
+
+            def copy_out():
+                copy(
+                    out=sgn[it][:, q0 * 512 : (q0 + n) * 512].bitcast(F32).rearrange("p (b i u) -> p b i u", b=n, u=2),
+                    in_=bank[:, 0 : n * 256].rearrange("p (b u i) -> p b i u", b=n, u=2),
+                )
+                give_bank(bank)
+
+            return copy_out
 
         def row_sums(s, halves=(0, 1)):
             it, g = s // GROUPS, s % GROUPS
-            if it not in wbank and summed_narrow(s):
-                wbank[it] = sump.tile([P, 512], F32, name="wbank")
             for v in halves:
                 for a in range(summed_narrow(s)):
                     k0 = v * P + (g * RG + a) * GROUP
                     for j in range(4):
                         c0 = a * N + j // 2 * 512 + v * 256
                         nc.tensor.matmul(
-                            wbank[it][:, k0 : k0 + GROUP],
+                            sums_bank[:, k0 : k0 + GROUP],
                             lhsT=grp[s][:, c0 + j % 2 : c0 + 256 : 2],
                             rhs=ones[:],
                             start=(j == 0),
                             stop=(j == 3),
                         )
 
+        def turned_sums(it):
+            return (sums_bank if it > 0 else first_sums)[:, 2 * P : 4 * P]
+
         def band_sum(s, a):
             it, r = s // GROUPS, s % GROUPS * RG + a
-            if s == 0 and a == 0:
-                sbank[0] = sump.tile([P, 512], F32, name="sbank")
             for c in range(2):
                 words = grp[s][:, a * N + c * 512 : a * N + (c + 1) * 512].rearrange("p (i u e) -> p u i e", u=2, e=2)
                 for u in range(2):
                     nc.tensor.matmul(
-                        sbank[it][:, 0 : 2 * P].rearrange("p (i e) -> p i e", e=2),
+                        turned_sums(it).rearrange("p (i e) -> p i e", e=2),
                         lhsT=band[:, P - GROUP * (r + 1) : 2 * P - GROUP * (r + 1)],
                         rhs=words[:, u],
                         start=(s == 0 and a == 0 and c == 0 and u == 0),
@@ -346,7 +367,7 @@ def tile_relationalgraphconvolution_pa_kernel(
 
         def keep_sums(it):
             dst = rep[patterns[it]][:, 0 : 2 * P].rearrange("p (v g m) -> p v g m", v=2, g=GROUPS)
-            src = wbank[it][:, 0 : 2 * P].rearrange("p (v g m) -> p v g m", v=2, g=GROUPS)
+            src = sums_bank[:, 0 : 2 * P].rearrange("p (v g m) -> p v g m", v=2, g=GROUPS)
             for g0, g1, (m, n) in runs_of(it):
                 if m:
                     nc.scalar.copy(out=dst[:, :, g0:g1, 0 : m * GROUP], in_=src[:, :, g0:g1, 0 : m * GROUP])
@@ -362,12 +383,10 @@ def tile_relationalgraphconvolution_pa_kernel(
                     )
 
         def turn_sums(it):
-            if it > 0:
-                sbank[it] = sump.tile([P, 512], F32, name="sbank")
             last = parts[patterns[it]] - 1
             for v in range(last + 1):
                 nc.tensor.matmul(
-                    sbank[it][:, v * P : (v + 1) * P] if v < 2 else sbank[it][:, 0 : 2 * P : 2],
+                    turned_sums(it)[:, v * P : (v + 1) * P] if v < 2 else turned_sums(it)[:, 0 : 2 * P : 2],
                     lhsT=rep[patterns[it]][:, v * P : (v + 1) * P],
                     rhs=ident[:],
                     start=(v == 0 and it > 0),
@@ -378,8 +397,10 @@ def tile_relationalgraphconvolution_pa_kernel(
         def collect_sums(it):
             sums[it] = two.tile([P, P], F32, name="sums", align_bytes=64)
             nc.vector.tensor_reduce(
-                out=sums[it][:], in_=sbank[it][:, 0 : 2 * P].rearrange("p (i u) -> p i u", u=2), axis=AXIS_X, op=ADD
+                out=sums[it][:], in_=turned_sums(it).rearrange("p (i u) -> p i u", u=2), axis=AXIS_X, op=ADD
             )
+            if it == 0:
+                give_bank(first_sums)
 
         def relation_part(it, engine):
             sgr[it] = two.tile([P, 1024], BF16, name="sgr", align_bytes=64)
@@ -404,7 +425,7 @@ def tile_relationalgraphconvolution_pa_kernel(
         def project(it, passes, first, last):
             for q in passes:
                 if q == first:
-                    obank[it] = ring.tile([P, 512], F32, name="bank")
+                    obank[it] = take_bank()
                 nc.tensor.matmul_mx(
                     out=obank[it][:, 0:NB],
                     lhsT=scodes[it][:, q * P : (q + 1) * P].bitcast(FP8X4),
@@ -415,9 +436,10 @@ def tile_relationalgraphconvolution_pa_kernel(
                     stop=(q == last),
                 )
 
-        def store(it):
+        def store(it, copy=nc.scalar.copy):
             res = three.tile([P, NB], F32, name="res", align_bytes=64)
-            nc.scalar.copy(out=res[:], in_=obank[it][:, 0:NB])
+            copy(out=res[:], in_=obank[it][:, 0:NB])
+            give_bank(obank[it])
             nc.sync.dma_start(out=out[0, it * P : (it + 1) * P, :], in_=res[:])
 
         def widen_weights(h, half):
@@ -431,7 +453,7 @@ def tile_relationalgraphconvolution_pa_kernel(
             )
 
         def turn_weights(q):
-            bank = ring.tile([P, 512], F32, name="bank")
+            bank = take_bank()
             for u in range(2):
                 for h in range(2):
                     k0 = (u * 2 + h) * P
@@ -439,10 +461,13 @@ def tile_relationalgraphconvolution_pa_kernel(
                     nc.tensor.transpose(bank[:, k0 : k0 + P], w_val[h][:].bitcast(F32)[:, w0 : w0 + P], ident[:])
             if q % 2 == 0:
                 w_grp[q // 2] = two.tile([P, 8 * NB], BF16, name="w_grp", align_bytes=64)
-            nc.scalar.copy(
-                out=w_grp[q // 2][:, q % 2 * 1024 : (q % 2 + 1) * 1024].bitcast(F32).rearrange("p (n u) -> p n u", u=2),
-                in_=bank[:].rearrange("p (u n) -> p n u", u=2),
-            )
+
+            def copy_out():
+                words = w_grp[q // 2][:, q % 2 * 1024 : (q % 2 + 1) * 1024].bitcast(F32)
+                nc.scalar.copy(out=words.rearrange("p (n u) -> p n u", u=2), in_=bank[:].rearrange("p (u n) -> p n u", u=2))
+                give_bank(bank)
+
+            return copy_out
 
         def scale_weights(q):
             values = w_grp[q // 2][:, q % 2 * 1024 : (q % 2 + 1) * 1024].rearrange("p (n t) -> p n t", t=4)
@@ -469,9 +494,13 @@ def tile_relationalgraphconvolution_pa_kernel(
         for s in range(3, PREFETCH):
             load(s, 2)
 
-        arrange(0)
-        nc.vector.tensor_reduce(out=pick[:], in_=ident[:].rearrange("p (g x) -> p x g", x=GROUP), axis=AXIS_X, op=ADD)
         to_clear = [key for key in rep if any(m < RG for m, n in key)]
+        for key in to_clear[:3]:
+            nc.vector.memset(rep[key][:], 0.0)
+        arrange(0)
+        for key in to_clear[3:]:
+            nc.vector.memset(rep[key][:], 0.0)
+        nc.vector.tensor_reduce(out=pick[:], in_=ident[:].rearrange("p (g x) -> p x g", x=GROUP), axis=AXIS_X, op=ADD)
         for s in range(STEPS - 1):
             it, phase = s // GROUPS - 1, s % GROUPS
             w = s - W_FROM
@@ -483,15 +512,22 @@ def tile_relationalgraphconvolution_pa_kernel(
             if s + PREFETCH < STEPS:
                 load(s + PREFETCH, 2 if s + PREFETCH <= HALVED else 1)
 
+            if s == STEPS - 2:
+                collect_sums(it)
+            window_first = it >= 0 and phase == 2 and s + 2 < STEPS
+            if window_first:
+                collect_sums(it)
+                relation_part(it, nc.gpsimd)
+                arrange(s + 2 if s > CATCH_UP else s + 1)
+            if 2 <= s <= CATCH_UP and not window_first:
+                arrange(s + 1)
             if s >= 1:
                 quantise(s - 1)
             if s - 1 in w_turn_at:
                 scale_weights(w_turn_at[s - 1])
-            if s < len(to_clear):
-                nc.vector.memset(rep[to_clear[s]][:], 0.0)
             if s == 0:
                 interleave_features()
-            if s <= CATCH_UP:
+            if s < 2:
                 arrange(s + 1)
             if s == 1:
                 quantise_features(0)
@@ -504,11 +540,10 @@ def tile_relationalgraphconvolution_pa_kernel(
                 pick_values(w_scale, scale_masked)
             if s in widen_at:
                 widen_weights(*divmod(widen_at.index(s), 2))
-            if it >= 0 and phase == 2:
-                collect_sums(it)
-                relation_part(it, nc.gpsimd if s + 2 < STEPS else nc.vector)
-            if CATCH_UP <= s < STEPS - 2:
+            if CATCH_UP <= s < STEPS - 2 and not window_first:
                 arrange(s + 2)
+            if s == STEPS - 2:
+                relation_part(it, nc.vector)
             if w_turn_at.get(s - 1, 0) % 2:
                 quantise_weights(w_turn_at[s - 1] // 2)
             if it >= 0 and phase == 3:
@@ -516,24 +551,32 @@ def tile_relationalgraphconvolution_pa_kernel(
             if it >= 1 and phase == 0:
                 quantise_supports(it - 1, 0, 4)
 
-            if it >= 0 and phase == 1:
-                keep_sums(it)
-                spread_sums(it)
-            for a in range(RG):
-                empty(s, a, turn(s, a))
-                if s == 0 and a in (1, 2):
-                    cross_features(a - 1)
-                k = RG * s + a - BAND_LAG
-                if 0 <= k < BAND_STEPS * RG and k % RG < 2:
-                    band_sum(k // RG, k % RG)
-            if it >= 0 and phase >= 2:
-                turn_supports(it, 2 * (phase - 2))
-            if s == STEPS - 2:
-                turn_supports(it, 2)
-            if it >= 0 and phase == 1:
-                turn_sums(it)
-            if s in w_turn_at:
-                turn_weights(w_turn_at[s])
+            if s <= BAND_STEPS:
+                for a in range(RG):
+                    empty(s, a, turn(s, a))
+                    if s == 0 and a >= 2:
+                        cross_features(a - 2)
+                    k = RG * s + a - BAND_LAG
+                    if 0 <= k < BAND_STEPS * RG and k % RG < 2:
+                        band_sum(k // RG, k % RG)
+            else:
+                banks = [turn(s, a) for a in range(RG)]
+                later = []
+                if it >= 0 and phase >= 2:
+                    later.append(turn_supports(it, 2 * (phase - 2)))
+                if s == STEPS - 2:
+                    later.append(turn_supports(it, 2))
+                if s in w_turn_at:
+                    later.append(turn_weights(w_turn_at[s]))
+                if it >= 0 and phase == 1:
+                    keep_sums(it)
+                    spread_sums(it)
+                empty(s, 1, banks[1])
+                empty(s, 0, banks[0])
+                for copy_out in reversed(later):
+                    copy_out()
+                empty(s, 3, banks[3])
+                empty(s, 2, banks[2])
             if s >= 1:
                 row_sums(s - 1, (0,))
             if s >= 2:
@@ -544,6 +587,8 @@ def tile_relationalgraphconvolution_pa_kernel(
                 store(project_at[s])
             if s >= 1:
                 row_sums(s - 1, (1,))
+            if it >= 0 and phase == 1:
+                turn_sums(it)
 
         s, it = STEPS - 1, IT - 1
         quantise(s - 1)
@@ -568,7 +613,7 @@ def tile_relationalgraphconvolution_pa_kernel(
         relation_part(it, nc.vector)
         project(it - 1, all_passes, 4, 3)
         for q in range(4):
-            turn_supports(it, q, 1)
+            turn_supports(it, q, 1)()
         store(it - 1)
         quantise_supports(it, 0, 1)
         quantise_supports(it, 4)

@@ -17,19 +17,22 @@ STEPS = IT * GROUPS
 GROUP = 8
 RUN = 16
 BANKS = 8
+NARROW, BAND, VECTOR = range(3)
 LEAD = 128
 PITCH = LEAD + N
 PASSES = F // 32
 PREFETCH = 5
 HALVED = 7
-W_FROM = 5
-ROWS_AT = 4
-V_UNTIL = 3
-V_FROM = 25
+W_FROM = 2
+ROWS_AT = 3
+V_UNTIL = 2
+V_FROM = 16
+WINDOW_FROM = 12
+EMPTY_FROM = 12
 BAND_STEPS = 2
 BAND_LAG = 3
 CATCH_UP = 7
-FIRST_PROJECT = W_FROM + 18
+FIRST_PROJECT = W_FROM + 13
 PROJECT_LAG = 9
 
 F32 = mybir.dt.float32
@@ -45,10 +48,20 @@ AXIS_X = mybir.AxisListType.X
 FLOPS = 2 * (R * N * N * DE + N * R * F * NB)
 
 
+def has_window(s):
+    return WINDOW_FROM <= s < STEPS - 2 and s % GROUPS == 2
+
+
 def summed_on_vector(s):
-    if s in (2 * GROUPS - 1, STEPS - 1) or (s > 2 * GROUPS and s % GROUPS == 0):
+    if s == STEPS - 1:
         return RG
-    return 2 if s < V_UNTIL or s >= V_FROM else 0
+    if has_window(s - 2):
+        return RG
+    return 2 if s < V_UNTIL or (s >= V_FROM and s % GROUPS == 3) else 0
+
+
+def vector_empties(s):
+    return int(s >= EMPTY_FROM and s % GROUPS == 2)
 
 
 def crossed(s):
@@ -57,6 +70,10 @@ def crossed(s):
 
 def summed_narrow(s):
     return crossed(s) if s >= BAND_STEPS else 0
+
+
+def summed_by(s, a):
+    return VECTOR if a >= crossed(s) else NARROW if summed_narrow(s) else BAND
 
 
 def tile_relationalgraphconvolution_pa_kernel(
@@ -69,18 +86,15 @@ def tile_relationalgraphconvolution_pa_kernel(
         onep = ctx.enter_context(tc.tile_pool(name="onep", bufs=8))
         two = ctx.enter_context(tc.tile_pool(name="two", bufs=2))
         three = ctx.enter_context(tc.tile_pool(name="three", bufs=3))
-        many = ctx.enter_context(tc.tile_pool(name="many", bufs=6))
+        many = ctx.enter_context(tc.tile_pool(name="many", bufs=4))
         psum = ctx.enter_context(tc.psum_pool(name="psum", bufs=1))
         ctx.enter_context(tc.manual_schedule())
 
         ident = keep.tile([P, P], F32, name="ident", align_bytes=64)
         make_identity(nc, ident[:])
         rs = keep.tile([P, STEPS * RG], F32, name="rs", align_bytes=64)
-        patterns = [
-            tuple((summed_narrow(s), summed_on_vector(s)) for s in range(GROUPS * it, GROUPS * (it + 1)))
-            for it in range(IT)
-        ]
-        parts = {key: 3 if any(n for m, n in key) else 2 for key in patterns}
+        patterns = [tuple(summed_by(GROUPS * it + r // RG, r % RG) for r in range(R)) for it in range(IT)]
+        parts = {key: 3 if VECTOR in key else 2 for key in patterns}
         rep = {}
         for key in patterns:
             if key not in rep:
@@ -245,17 +259,23 @@ def tile_relationalgraphconvolution_pa_kernel(
             )
 
         def arrange(s):
+            cross_tiles(s)
+            sum_tiles(s)
+
+        def sum_tiles(s):
+            for a in range(crossed(s), RG):
+                sort_and_sum(s, a)
+
+        def cross_tiles(s):
             n = crossed(s)
             if s == 0:
-                cross(s, 0, 1)
-                cross(s, 1, 1)
+                for a in range(n):
+                    cross(s, a, 1)
             elif n == RG and s <= HALVED:
                 cross(s, 0, 2)
                 cross(s, 2, 2)
             elif n:
                 cross(s, 0, n)
-            for a in range(n, RG):
-                sort_and_sum(s, a)
 
         def turn(s, a):
             if a == 0:
@@ -273,7 +293,6 @@ def tile_relationalgraphconvolution_pa_kernel(
                 out=grp[s][:, a * N : (a + 1) * N].bitcast(F32).rearrange("p (c i u) -> p c i u", c=2, u=2),
                 in_=bank[:].rearrange("p (c u i) -> p c i u", c=2, u=2),
             )
-            give_bank(bank)
 
         def quantise(s, a0=0, n=RG):
             if a0 == 0:
@@ -360,27 +379,24 @@ def tile_relationalgraphconvolution_pa_kernel(
                         stop=False,
                     )
 
-        def runs_of(it):
-            key = patterns[it]
-            starts = [g for g in range(GROUPS) if g == 0 or key[g] != key[g - 1]]
-            return [(g0, g1, key[g0]) for g0, g1 in zip(starts, starts[1:] + [GROUPS])]
+        def runs_of(it, kind):
+            marks = [0] + [int(k == kind) for k in patterns[it]] + [0]
+            starts = [r for r in range(R) if marks[r + 1] > marks[r]]
+            return zip(starts, [r for r in range(1, R + 1) if marks[r + 1] < marks[r]])
 
         def keep_sums(it):
-            dst = rep[patterns[it]][:, 0 : 2 * P].rearrange("p (v g m) -> p v g m", v=2, g=GROUPS)
-            src = sums_bank[:, 0 : 2 * P].rearrange("p (v g m) -> p v g m", v=2, g=GROUPS)
-            for g0, g1, (m, n) in runs_of(it):
-                if m:
-                    nc.scalar.copy(out=dst[:, :, g0:g1, 0 : m * GROUP], in_=src[:, :, g0:g1, 0 : m * GROUP])
+            dst = rep[patterns[it]][:, 0 : 2 * P].rearrange("p (v m) -> p v m", v=2)
+            src = sums_bank[:, 0 : 2 * P].rearrange("p (v m) -> p v m", v=2)
+            for r0, r1 in runs_of(it, NARROW):
+                nc.scalar.copy(out=dst[:, :, r0 * GROUP : r1 * GROUP], in_=src[:, :, r0 * GROUP : r1 * GROUP])
 
         def spread_sums(it):
-            for g0, g1, (m, n) in runs_of(it):
-                if n:
-                    dst = rep[patterns[it]][:, 2 * P : 3 * P].rearrange("p (g a x) -> p g a x", g=GROUPS, x=GROUP)
-                    src = rs[:, it * R : (it + 1) * R].rearrange("p (g a) -> p g a", a=RG)
-                    nc.scalar.copy(
-                        out=dst[:, g0:g1, RG - n :, :],
-                        in_=src[:, g0:g1, RG - n :].unsqueeze(3).to_broadcast([P, g1 - g0, n, GROUP]),
-                    )
+            for r0, r1 in runs_of(it, VECTOR):
+                dst = rep[patterns[it]][:, 2 * P + r0 * GROUP : 2 * P + r1 * GROUP]
+                nc.scalar.copy(
+                    out=dst.rearrange("p (r x) -> p r x", x=GROUP),
+                    in_=rs[:, it * R + r0 : it * R + r1].unsqueeze(2).to_broadcast([P, r1 - r0, GROUP]),
+                )
 
         def turn_sums(it):
             last = parts[patterns[it]] - 1
@@ -484,19 +500,25 @@ def tile_relationalgraphconvolution_pa_kernel(
 
         all_passes = (4, 5, 0, 1, 2, 3)
         project_at = {max(GROUPS * it + PROJECT_LAG, it + FIRST_PROJECT): it for it in range(IT)}
-        w_turn_at = {W_FROM + 5 + 2 * q: q for q in range(PASSES)}
-        widen_at = [s for s in range(W_FROM, W_FROM + 5) if s % GROUPS != 2]
+        w_turn_at = {W_FROM + 4 + q: q for q in range(PASSES)}
 
-        load(0, 4)
         load_features()
+        load(0, 4)
         load(1, 2)
         load(2, 2)
-        for s in range(3, PREFETCH):
+        nc.sync.dma_start(out=w_bytes[0][:], in_=Wb_bytes[0:P, :])
+        load(3, 2)
+        nc.sync.dma_start(out=w_bytes[1][:], in_=Wb_bytes[P : 2 * P, :])
+        load_rows(scale_rows, Wb_scale.rearrange("o (r f) -> (o r) f", f=F))
+        load_rows(rel_rows, relation_features[0])
+        for s in range(4, PREFETCH):
             load(s, 2)
 
-        to_clear = [key for key in rep if any(m < RG for m, n in key)]
+        to_clear = [key for key in rep if key.count(NARROW) < R]
         for key in to_clear[:3]:
             nc.vector.memset(rep[key][:], 0.0)
+        cross_features(0)
+        cross_features(1)
         arrange(0)
         for key in to_clear[3:]:
             nc.vector.memset(rep[key][:], 0.0)
@@ -504,33 +526,47 @@ def tile_relationalgraphconvolution_pa_kernel(
         for s in range(STEPS - 1):
             it, phase = s // GROUPS - 1, s % GROUPS
             w = s - W_FROM
-            if w in (-4, -3):
-                nc.sync.dma_start(out=w_bytes[w + 4][:], in_=Wb_bytes[(w + 4) * P : (w + 5) * P, :])
-            if s == 0:
-                load_rows(rel_rows, relation_features[0])
-                load_rows(scale_rows, Wb_scale.rearrange("o (r f) -> (o r) f", f=F))
             if s + PREFETCH < STEPS:
                 load(s + PREFETCH, 2 if s + PREFETCH <= HALVED else 1)
 
-            if s == STEPS - 2:
+            banks, later = [], []
+            if s > BAND_STEPS:
+                banks = [turn(s, a) for a in range(RG)]
+                if it >= 0 and phase >= 2:
+                    later.append(turn_supports(it, 2 * (phase - 2)))
+                if s == STEPS - 2:
+                    later.append(turn_supports(it, 2))
+                if s in w_turn_at:
+                    later.append(turn_weights(w_turn_at[s]))
+
+            on_vector = it >= 0 and phase == 2 and not has_window(s)
+            if on_vector:
                 collect_sums(it)
-            window_first = it >= 0 and phase == 2 and s + 2 < STEPS
-            if window_first:
+            ahead = s + 2 if s > CATCH_UP else s + 1
+            by_vector = range(RG - vector_empties(s), RG)
+            if has_window(s):
                 collect_sums(it)
                 relation_part(it, nc.gpsimd)
-                arrange(s + 2 if s > CATCH_UP else s + 1)
-            if 2 <= s <= CATCH_UP and not window_first:
+                sum_tiles(ahead)
+                for a in by_vector:
+                    empty(s, a, banks[a], nc.vector.tensor_copy)
+                cross_tiles(ahead)
+            elif 2 <= s <= CATCH_UP:
                 arrange(s + 1)
             if s >= 1:
                 quantise(s - 1)
+            if not has_window(s):
+                for a in by_vector:
+                    empty(s, a, banks[a], nc.vector.tensor_copy)
             if s - 1 in w_turn_at:
                 scale_weights(w_turn_at[s - 1])
             if s == 0:
                 interleave_features()
             if s < 2:
                 arrange(s + 1)
-            if s == 1:
+            if s == 0:
                 quantise_features(0)
+            if s == 1:
                 quantise_features(1)
             if s == ROWS_AT:
                 mask_rows(rel_masked, rel_rows, DR)
@@ -538,45 +574,38 @@ def tile_relationalgraphconvolution_pa_kernel(
             if s == ROWS_AT + 1:
                 pick_values(relf, rel_masked)
                 pick_values(w_scale, scale_masked)
-            if s in widen_at:
-                widen_weights(*divmod(widen_at.index(s), 2))
-            if CATCH_UP <= s < STEPS - 2 and not window_first:
+            if 0 <= w < 4:
+                widen_weights(w // 2, w % 2)
+            if s == CATCH_UP or (CATCH_UP < s < STEPS - 2 and not has_window(s)):
                 arrange(s + 2)
-            if s == STEPS - 2:
+            if on_vector:
                 relation_part(it, nc.vector)
-            if w_turn_at.get(s - 1, 0) % 2:
-                quantise_weights(w_turn_at[s - 1] // 2)
+            if w_turn_at.get(s - 2, 0) % 2:
+                quantise_weights(w_turn_at[s - 2] // 2)
             if it >= 0 and phase == 3:
                 quantise_supports(it, 4)
             if it >= 1 and phase == 0:
                 quantise_supports(it - 1, 0, 4)
 
+            if it >= 0 and phase == 1:
+                keep_sums(it)
+                spread_sums(it)
             if s <= BAND_STEPS:
                 for a in range(RG):
-                    empty(s, a, turn(s, a))
-                    if s == 0 and a >= 2:
-                        cross_features(a - 2)
+                    bank = turn(s, a)
+                    empty(s, a, bank)
+                    give_bank(bank)
                     k = RG * s + a - BAND_LAG
                     if 0 <= k < BAND_STEPS * RG and k % RG < 2:
                         band_sum(k // RG, k % RG)
             else:
-                banks = [turn(s, a) for a in range(RG)]
-                later = []
-                if it >= 0 and phase >= 2:
-                    later.append(turn_supports(it, 2 * (phase - 2)))
-                if s == STEPS - 2:
-                    later.append(turn_supports(it, 2))
-                if s in w_turn_at:
-                    later.append(turn_weights(w_turn_at[s]))
-                if it >= 0 and phase == 1:
-                    keep_sums(it)
-                    spread_sums(it)
-                empty(s, 1, banks[1])
-                empty(s, 0, banks[0])
-                for copy_out in reversed(later):
-                    copy_out()
-                empty(s, 3, banks[3])
-                empty(s, 2, banks[2])
+                for a in range(RG - vector_empties(s)):
+                    empty(s, a, banks[a])
+                    give_bank(banks[a])
+            for copy_out in later:
+                copy_out()
+            for a in by_vector:
+                give_bank(banks[a])
             if s >= 1:
                 row_sums(s - 1, (0,))
             if s >= 2:
@@ -595,7 +624,9 @@ def tile_relationalgraphconvolution_pa_kernel(
         quantise_supports(it - 1, 0, 4)
         quantise_supports(it - 1, 4)
         for a in range(RG):
-            empty(s, a, turn(s, a), nc.vector.tensor_copy if a == 3 else nc.scalar.copy)
+            bank = turn(s, a)
+            empty(s, a, bank, nc.vector.tensor_copy if a == 3 else nc.scalar.copy)
+            give_bank(bank)
         row_sums(s - 1)
         keep_sums(it)
         spread_sums(it)

@@ -23,16 +23,16 @@ PITCH = LEAD + N
 PASSES = F // 32
 PREFETCH = 5
 HALVED = 7
-W_FROM = 2
-ROWS_AT = 3
-V_UNTIL = 2
+W_FROM = 6
+ROWS_AT = 4
+V_UNTIL = 6
 V_FROM = 16
-WINDOW_FROM = 12
-EMPTY_FROM = 12
+WINDOW_FROM = 18
+EMPTY_FROM = 32
 BAND_STEPS = 2
 BAND_LAG = 3
 CATCH_UP = 7
-FIRST_PROJECT = W_FROM + 13
+FIRST_PROJECT = W_FROM + 14
 PROJECT_LAG = 9
 
 F32 = mybir.dt.float32
@@ -86,7 +86,7 @@ def tile_relationalgraphconvolution_pa_kernel(
         onep = ctx.enter_context(tc.tile_pool(name="onep", bufs=8))
         two = ctx.enter_context(tc.tile_pool(name="two", bufs=2))
         three = ctx.enter_context(tc.tile_pool(name="three", bufs=3))
-        many = ctx.enter_context(tc.tile_pool(name="many", bufs=4))
+        many = ctx.enter_context(tc.tile_pool(name="many", bufs=5))
         psum = ctx.enter_context(tc.psum_pool(name="psum", bufs=1))
         ctx.enter_context(tc.manual_schedule())
 
@@ -500,25 +500,16 @@ def tile_relationalgraphconvolution_pa_kernel(
 
         all_passes = (4, 5, 0, 1, 2, 3)
         project_at = {max(GROUPS * it + PROJECT_LAG, it + FIRST_PROJECT): it for it in range(IT)}
-        w_turn_at = {W_FROM + 4 + q: q for q in range(PASSES)}
+        w_turn_at = {W_FROM + 4 + 3 * q // 2: q for q in range(PASSES)}
 
-        load_features()
         load(0, 4)
-        load(1, 2)
-        load(2, 2)
-        nc.sync.dma_start(out=w_bytes[0][:], in_=Wb_bytes[0:P, :])
-        load(3, 2)
-        nc.sync.dma_start(out=w_bytes[1][:], in_=Wb_bytes[P : 2 * P, :])
-        load_rows(scale_rows, Wb_scale.rearrange("o (r f) -> (o r) f", f=F))
-        load_rows(rel_rows, relation_features[0])
-        for s in range(4, PREFETCH):
+        load_features()
+        for s in range(1, PREFETCH):
             load(s, 2)
 
         to_clear = [key for key in rep if key.count(NARROW) < R]
         for key in to_clear[:3]:
             nc.vector.memset(rep[key][:], 0.0)
-        cross_features(0)
-        cross_features(1)
         arrange(0)
         for key in to_clear[3:]:
             nc.vector.memset(rep[key][:], 0.0)
@@ -526,6 +517,12 @@ def tile_relationalgraphconvolution_pa_kernel(
         for s in range(STEPS - 1):
             it, phase = s // GROUPS - 1, s % GROUPS
             w = s - W_FROM
+            if s == 0:
+                load_rows(rel_rows, relation_features[0])
+            if w in (-4, -3):
+                nc.sync.dma_start(out=w_bytes[w + 4][:], in_=Wb_bytes[(w + 4) * P : (w + 5) * P, :])
+            if w == -2:
+                load_rows(scale_rows, Wb_scale.rearrange("o (r f) -> (o r) f", f=F))
             if s + PREFETCH < STEPS:
                 load(s + PREFETCH, 2 if s + PREFETCH <= HALVED else 1)
 
@@ -570,9 +567,11 @@ def tile_relationalgraphconvolution_pa_kernel(
                 quantise_features(1)
             if s == ROWS_AT:
                 mask_rows(rel_masked, rel_rows, DR)
-                mask_rows(scale_masked, scale_rows, F)
             if s == ROWS_AT + 1:
                 pick_values(relf, rel_masked)
+            if w == 3:
+                mask_rows(scale_masked, scale_rows, F)
+            if w == 4:
                 pick_values(w_scale, scale_masked)
             if 0 <= w < 4:
                 widen_weights(w // 2, w % 2)
@@ -595,6 +594,8 @@ def tile_relationalgraphconvolution_pa_kernel(
                     bank = turn(s, a)
                     empty(s, a, bank)
                     give_bank(bank)
+                    if s == 0 and a >= 2:
+                        cross_features(a - 2)
                     k = RG * s + a - BAND_LAG
                     if 0 <= k < BAND_STEPS * RG and k % RG < 2:
                         band_sum(k // RG, k % RG)

@@ -25,9 +25,10 @@ PREFETCH = 5
 HALVED = 7
 W_FROM = 6
 ROWS_AT = 4
-V_UNTIL = 6
-V_FROM = 16
+V_UNTIL = 4
+V_FROM = 20
 WINDOW_FROM = 18
+CATCHING_UP = 25
 EMPTY_FROM = 32
 BAND_STEPS = 2
 BAND_LAG = 3
@@ -57,7 +58,7 @@ def summed_on_vector(s):
         return RG
     if has_window(s - 2):
         return RG
-    return 2 if s < V_UNTIL or (s >= V_FROM and s % GROUPS == 3) else 0
+    return 2 if s < V_UNTIL or (s >= V_FROM and s % GROUPS == 3) or s == CATCHING_UP else 0
 
 
 def vector_empties(s):
@@ -519,9 +520,9 @@ def tile_relationalgraphconvolution_pa_kernel(
             w = s - W_FROM
             if s == 0:
                 load_rows(rel_rows, relation_features[0])
-            if w in (-4, -3):
-                nc.sync.dma_start(out=w_bytes[w + 4][:], in_=Wb_bytes[(w + 4) * P : (w + 5) * P, :])
-            if w == -2:
+            if w in (-3, -2):
+                nc.sync.dma_start(out=w_bytes[w + 3][:], in_=Wb_bytes[(w + 3) * P : (w + 4) * P, :])
+            if w == 0:
                 load_rows(scale_rows, Wb_scale.rearrange("o (r f) -> (o r) f", f=F))
             if s + PREFETCH < STEPS:
                 load(s + PREFETCH, 2 if s + PREFETCH <= HALVED else 1)

@@ -17,6 +17,7 @@ STEPS = IT * GROUPS
 GROUP = 8
 RUN = 16
 BANKS = 8
+EDGE = 4
 NARROW, BAND, VECTOR = range(3)
 LEAD = 128
 PITCH = LEAD + N
@@ -306,9 +307,11 @@ def tile_relationalgraphconvolution_pa_kernel(
                 in_=grp[s][:, a0 * N : (a0 + n) * N],
             )
 
-        def aggregate(s, a0=0, n=RG):
+        def aggregate(s, a0=0, n=RG, between=None):
             mx[s, a0] = take_bank()
             for a in range(a0, a0 + n):
+                if between and a == RG // 2:
+                    issue(between, len(between) - EDGE)
                 for c in range(2):
                     cols = slice(a * 256 + c * P, a * 256 + (c + 1) * P)
                     f0 = (c + 2 * (a < crossed(s))) * DE
@@ -349,20 +352,25 @@ def tile_relationalgraphconvolution_pa_kernel(
 
             return copy_out
 
-        def row_sums(s, halves=(0, 1)):
-            it, g = s // GROUPS, s % GROUPS
-            for v in halves:
-                for a in range(summed_narrow(s)):
-                    k0 = v * P + (g * RG + a) * GROUP
-                    for j in range(4):
-                        c0 = a * N + j // 2 * 512 + v * 256
-                        nc.tensor.matmul(
-                            sums_bank[:, k0 : k0 + GROUP],
-                            lhsT=grp[s][:, c0 + j % 2 : c0 + 256 : 2],
-                            rhs=ones[:],
-                            start=(j == 0),
-                            stop=(j == 3),
-                        )
+        def narrow_sum(s, a, v, j):
+            k0 = v * P + (s % GROUPS * RG + a) * GROUP
+            c0 = a * N + j // 2 * 512 + v * 256
+            nc.tensor.matmul(
+                sums_bank[:, k0 : k0 + GROUP],
+                lhsT=grp[s][:, c0 + j % 2 : c0 + 256 : 2],
+                rhs=ones[:],
+                start=(j == 0),
+                stop=(j == 3),
+            )
+
+        def narrow_sums(s):
+            return [(s, a, v, j) for v in range(2) for a in range(summed_narrow(s)) for j in range(4)]
+
+        def issue(narrow, n):
+            n = max(n, 0)
+            for item in narrow[:n]:
+                narrow_sum(*item)
+            narrow[:n] = []
 
         def turned_sums(it):
             return (sums_bank if it > 0 else first_sums)[:, 2 * P : 4 * P]
@@ -608,16 +616,16 @@ def tile_relationalgraphconvolution_pa_kernel(
                 copy_out()
             for a in by_vector:
                 give_bank(banks[a])
-            if s >= 1:
-                row_sums(s - 1, (0,))
+            narrow = narrow_sums(s - 1) if s >= 1 else []
+            short = not later and s not in project_at
+            issue(narrow, EDGE if short else len(narrow) // 2)
             if s >= 2:
-                aggregate(s - 2)
+                aggregate(s - 2, between=narrow if short else None)
                 keep_supports(s - 2)
             if s in project_at:
                 project(project_at[s], all_passes, 4, 3)
                 store(project_at[s])
-            if s >= 1:
-                row_sums(s - 1, (1,))
+            issue(narrow, len(narrow))
             if it >= 0 and phase == 1:
                 turn_sums(it)
 
@@ -629,11 +637,13 @@ def tile_relationalgraphconvolution_pa_kernel(
             bank = turn(s, a)
             empty(s, a, bank, nc.vector.tensor_copy if a == 3 else nc.scalar.copy)
             give_bank(bank)
-        row_sums(s - 1)
+        narrow = narrow_sums(s - 1)
+        issue(narrow, EDGE)
+        aggregate(s - 2)
+        issue(narrow, len(narrow))
+        keep_supports(s - 2)
         keep_sums(it)
         spread_sums(it)
-        aggregate(s - 2)
-        keep_supports(s - 2)
         aggregate(s - 1)
         keep_supports(s - 1)
         turn_sums(it)

@@ -617,7 +617,7 @@ def tile_relationalgraphconvolution_pa_kernel(
             for a in by_vector:
                 give_bank(banks[a])
             narrow = narrow_sums(s - 1) if s >= 1 else []
-            short = not later and s not in project_at
+            short = s not in project_at
             issue(narrow, EDGE if short else len(narrow) // 2)
             if s >= 2:
                 aggregate(s - 2, between=narrow if short else None)

@@ -14,6 +14,7 @@ IT = N // P
 RG = 4
 GROUPS = R // RG
 STEPS = IT * GROUPS
+GROUP_AT = (0, 2, 1, 3)
 GROUP = 8
 RUN = 16
 BANKS = 8
@@ -24,18 +25,26 @@ PITCH = LEAD + N
 PASSES = F // 32
 PREFETCH = 5
 HALVED = 7
-W_FROM = 6
-ROWS_AT = 4
-V_UNTIL = 4
-V_FROM = 20
-WINDOW_FROM = 18
-CATCHING_UP = 25
-EMPTY_FROM = 32
-BAND_STEPS = 2
-BAND_LAG = 3
-CATCH_UP = 7
-FIRST_PROJECT = W_FROM + 14
-PROJECT_LAG = 9
+W_FIRST = 9
+W_AHEAD = 1
+WEAVE = 0
+W_LOAD = (0, 2)
+WIDEN_AT = (3, 3, 5, 5)
+FEATURES_FIRST = 1
+EARLY = 5
+BAND_UNTIL = 2
+BAND_AT = (4, 7, 10, 11)
+CROSS_AT = (6, 7)
+CATCH_UP = 8
+SPREADS = 4
+MANY = 5
+BAND_STEPS = 1
+EXTRA_V = {}
+PROJECT_AT = (19, 21, 23, 25, 27, 29)
+SWAP = 1
+SPLIT_FROM = 4
+PROJECT_EVERY = 2
+EMPTY_AT = range(W_FIRST - 1, W_FIRST + 2 * PASSES - 1, 2)
 
 F32 = mybir.dt.float32
 BF16 = mybir.dt.bfloat16
@@ -50,32 +59,20 @@ AXIS_X = mybir.AxisListType.X
 FLOPS = 2 * (R * N * N * DE + N * R * F * NB)
 
 
-def has_window(s):
-    return WINDOW_FROM <= s < STEPS - 2 and s % GROUPS == 2
+def first_relation(s):
+    return GROUP_AT[s % GROUPS] * RG
 
 
-def summed_on_vector(s):
-    if s == STEPS - 1:
-        return RG
-    if has_window(s - 2):
-        return RG
-    return 2 if s < V_UNTIL or (s >= V_FROM and s % GROUPS == 3) or s == CATCHING_UP else 0
-
-
-def vector_empties(s):
-    return int(s >= EMPTY_FROM and s % GROUPS == 2)
-
-
-def crossed(s):
-    return RG - summed_on_vector(s)
-
-
-def summed_narrow(s):
-    return crossed(s) if s >= BAND_STEPS else 0
+def on_vector(s):
+    if s % 2 and s >= W_FIRST - 2:
+        return RG - (s - 1 in EMPTY_AT and SWAP)
+    return EXTRA_V.get(s, 0)
 
 
 def summed_by(s, a):
-    return VECTOR if a >= crossed(s) else NARROW if summed_narrow(s) else BAND
+    if a >= RG - on_vector(s):
+        return VECTOR
+    return BAND if s == 0 else NARROW
 
 
 def tile_relationalgraphconvolution_pa_kernel(
@@ -88,19 +85,15 @@ def tile_relationalgraphconvolution_pa_kernel(
         onep = ctx.enter_context(tc.tile_pool(name="onep", bufs=8))
         two = ctx.enter_context(tc.tile_pool(name="two", bufs=2))
         three = ctx.enter_context(tc.tile_pool(name="three", bufs=3))
-        many = ctx.enter_context(tc.tile_pool(name="many", bufs=5))
+        many = ctx.enter_context(tc.tile_pool(name="many", bufs=MANY))
         psum = ctx.enter_context(tc.psum_pool(name="psum", bufs=1))
         ctx.enter_context(tc.manual_schedule())
 
         ident = keep.tile([P, P], F32, name="ident", align_bytes=64)
         make_identity(nc, ident[:])
         rs = keep.tile([P, STEPS * RG], F32, name="rs", align_bytes=64)
-        patterns = [tuple(summed_by(GROUPS * it + r // RG, r % RG) for r in range(R)) for it in range(IT)]
-        parts = {key: 3 if VECTOR in key else 2 for key in patterns}
-        rep = {}
-        for key in patterns:
-            if key not in rep:
-                rep[key] = keep.tile([P, parts[key] * P], F32, name="rep%d" % len(rep), align_bytes=64)
+        kinds = [[summed_by(GROUPS * it + GROUP_AT.index(r // RG), r % RG) for r in range(R)] for it in range(IT)]
+        rep = [keep.tile([P, 3 * P], F32, name="rep%d" % it, align_bytes=64) for it in range(IT)]
         ones = keep.tile([P, GROUP], BF16, name="ones", align_bytes=64)
         nc.vector.memset(ones[:], 1.0)
         band = keep.tile([P, 2 * P - GROUP], BF16, name="band", align_bytes=64)
@@ -161,16 +154,17 @@ def tile_relationalgraphconvolution_pa_kernel(
         sums_bank = psum.tile([P, 512], F32, name="bank%d" % (BANKS - 1))
         first_sums = psum.tile([P, 512], F32, name="bank%d" % (BANKS - 2))
         held[BANKS - 2] = first_sums
+        turned = {0: first_sums}
 
         def rows_of(s, a0, n, first):
             return raw[s][:, first + a0 * PITCH : first + (a0 + n) * PITCH].rearrange("p (a q) -> p a q", q=PITCH)
 
         def load(s, pieces=1):
-            it, g = s // GROUPS, s % GROUPS
+            it = s // GROUPS
             raw[s] = rawp.tile([P, LEAD + RG * PITCH], BF16, name="raw", align_bytes=256)
             n = RG // pieces
             for a0 in range(0, RG, n):
-                r0 = g * RG + a0
+                r0 = first_relation(s) + a0
                 nc.sync.dma_start(
                     out=rows_of(s, a0, n, LEAD)[:, :, 0:N],
                     in_=adj[0, r0 : r0 + n, it * P : (it + 1) * P, :].rearrange("r i j -> i r j"),
@@ -225,10 +219,10 @@ def tile_relationalgraphconvolution_pa_kernel(
                 op=MULT,
             )
 
-        def pick_values(dst, masked):
+        def pick_values(dst, masked, q0, n):
             nc.vector.tensor_reduce(
-                out=dst[:].rearrange("p (m e) -> p m e", e=2),
-                in_=masked[:].rearrange("p (m x e) -> p m e x", x=GROUP, e=2),
+                out=dst[:, q0 * 4 : (q0 + n) * 4].rearrange("p (m e) -> p m e", e=2),
+                in_=masked[:, q0 * 32 : (q0 + n) * 32].rearrange("p (m x e) -> p m e x", x=GROUP, e=2),
                 axis=AXIS_X,
                 op=ADD,
             )
@@ -247,6 +241,7 @@ def tile_relationalgraphconvolution_pa_kernel(
             nc.vector.tensor_copy(out=dst, in_=src)
 
         def sort_and_sum(s, a):
+            k = s // GROUPS * R + first_relation(s) + a
             dst = onep.tile([P, N], BF16, name="sorted", align_bytes=64)
             for c in range(2):
                 window[s, a, c] = [(dst, (2 * u + c) * P) for u in range(2)]
@@ -257,27 +252,8 @@ def tile_relationalgraphconvolution_pa_kernel(
                 scalar2=None,
                 op0=MULT,
                 op1=ADD,
-                accum_out=rs[:, s * RG + a : s * RG + a + 1],
+                accum_out=rs[:, k : k + 1],
             )
-
-        def arrange(s):
-            cross_tiles(s)
-            sum_tiles(s)
-
-        def sum_tiles(s):
-            for a in range(crossed(s), RG):
-                sort_and_sum(s, a)
-
-        def cross_tiles(s):
-            n = crossed(s)
-            if s == 0:
-                for a in range(n):
-                    cross(s, a, 1)
-            elif n == RG and s <= HALVED:
-                cross(s, 0, 2)
-                cross(s, 2, 2)
-            elif n:
-                cross(s, 0, n)
 
         def turn(s, a):
             if a == 0:
@@ -307,14 +283,16 @@ def tile_relationalgraphconvolution_pa_kernel(
                 in_=grp[s][:, a0 * N : (a0 + n) * N],
             )
 
-        def aggregate(s, a0=0, n=RG, between=None):
-            mx[s, a0] = take_bank()
-            for a in range(a0, a0 + n):
-                if between and a == RG // 2:
-                    issue(between, len(between) - EDGE)
+        def aggregate_half(s, half):
+            aggregate(s, 0, RG, range(2 * half, 2 * half + 2))
+
+        def aggregate(s, a0=0, n=RG, tiles=None):
+            if (s, a0) not in mx:
+                mx[s, a0] = take_bank()
+            for a in tiles or range(a0, a0 + n):
                 for c in range(2):
                     cols = slice(a * 256 + c * P, a * 256 + (c + 1) * P)
-                    f0 = (c + 2 * (a < crossed(s))) * DE
+                    f0 = (c + 2 * (summed_by(s, a) != VECTOR)) * DE
                     nc.tensor.matmul_mx(
                         out=mx[s, a0][:, (a - a0) * DE : (a - a0 + 1) * DE],
                         lhsT=codes[s][:, cols].bitcast(FP8X4),
@@ -326,7 +304,7 @@ def tile_relationalgraphconvolution_pa_kernel(
                     )
 
         def keep_supports(s, a0=0, n=RG):
-            it, r0 = s // GROUPS, s % GROUPS * RG + a0
+            it, r0 = s // GROUPS, first_relation(s) + a0
             if r0 == 0:
                 supn[it] = two.tile([P, R * DE], BF16, name="supn", align_bytes=64)
             nc.scalar.copy(
@@ -353,7 +331,7 @@ def tile_relationalgraphconvolution_pa_kernel(
             return copy_out
 
         def narrow_sum(s, a, v, j):
-            k0 = v * P + (s % GROUPS * RG + a) * GROUP
+            k0 = v * P + (first_relation(s) + a) * GROUP
             c0 = a * N + j // 2 * 512 + v * 256
             nc.tensor.matmul(
                 sums_bank[:, k0 : k0 + GROUP],
@@ -363,9 +341,6 @@ def tile_relationalgraphconvolution_pa_kernel(
                 stop=(j == 3),
             )
 
-        def narrow_sums(s):
-            return [(s, a, v, j) for v in range(2) for a in range(summed_narrow(s)) for j in range(4)]
-
         def issue(narrow, n):
             n = max(n, 0)
             for item in narrow[:n]:
@@ -373,10 +348,10 @@ def tile_relationalgraphconvolution_pa_kernel(
             narrow[:n] = []
 
         def turned_sums(it):
-            return (sums_bank if it > 0 else first_sums)[:, 2 * P : 4 * P]
+            return turned[it][:, 0 : 2 * P]
 
         def band_sum(s, a):
-            it, r = s // GROUPS, s % GROUPS * RG + a
+            it, r = s // GROUPS, first_relation(s) + a
             for c in range(2):
                 words = grp[s][:, a * N + c * 512 : a * N + (c + 1) * 512].rearrange("p (i u e) -> p u i e", u=2, e=2)
                 for u in range(2):
@@ -388,31 +363,33 @@ def tile_relationalgraphconvolution_pa_kernel(
                         stop=False,
                     )
 
-        def runs_of(it, kind):
-            marks = [0] + [int(k == kind) for k in patterns[it]] + [0]
+        def columns_of(it, kind):
+            marks = [0] + [int(k == kind) for k in kinds[it]] + [0]
             starts = [r for r in range(R) if marks[r + 1] > marks[r]]
             return zip(starts, [r for r in range(1, R + 1) if marks[r + 1] < marks[r]])
 
         def keep_sums(it):
-            dst = rep[patterns[it]][:, 0 : 2 * P].rearrange("p (v m) -> p v m", v=2)
+            dst = rep[it][:, 0 : 2 * P].rearrange("p (v m) -> p v m", v=2)
             src = sums_bank[:, 0 : 2 * P].rearrange("p (v m) -> p v m", v=2)
-            for r0, r1 in runs_of(it, NARROW):
+            for r0, r1 in columns_of(it, NARROW):
                 nc.scalar.copy(out=dst[:, :, r0 * GROUP : r1 * GROUP], in_=src[:, :, r0 * GROUP : r1 * GROUP])
 
         def spread_sums(it):
-            for r0, r1 in runs_of(it, VECTOR):
-                dst = rep[patterns[it]][:, 2 * P + r0 * GROUP : 2 * P + r1 * GROUP]
+            for r0, r1 in columns_of(it, VECTOR):
+                dst = rep[it][:, 2 * P + r0 * GROUP : 2 * P + r1 * GROUP]
                 nc.scalar.copy(
                     out=dst.rearrange("p (r x) -> p r x", x=GROUP),
                     in_=rs[:, it * R + r0 : it * R + r1].unsqueeze(2).to_broadcast([P, r1 - r0, GROUP]),
                 )
 
         def turn_sums(it):
-            last = parts[patterns[it]] - 1
+            last = 2 if VECTOR in kinds[it] else 1
+            if it > 0:
+                turned[it] = take_bank()
             for v in range(last + 1):
                 nc.tensor.matmul(
                     turned_sums(it)[:, v * P : (v + 1) * P] if v < 2 else turned_sums(it)[:, 0 : 2 * P : 2],
-                    lhsT=rep[patterns[it]][:, v * P : (v + 1) * P],
+                    lhsT=rep[it][:, v * P : (v + 1) * P],
                     rhs=ident[:],
                     start=(v == 0 and it > 0),
                     stop=(v == last),
@@ -424,8 +401,7 @@ def tile_relationalgraphconvolution_pa_kernel(
             nc.vector.tensor_reduce(
                 out=sums[it][:], in_=turned_sums(it).rearrange("p (i u) -> p i u", u=2), axis=AXIS_X, op=ADD
             )
-            if it == 0:
-                give_bank(first_sums)
+            give_bank(turned[it])
 
         def relation_part(it, engine):
             sgr[it] = two.tile([P, 1024], BF16, name="sgr", align_bytes=64)
@@ -484,150 +460,188 @@ def tile_relationalgraphconvolution_pa_kernel(
                     k0 = (u * 2 + h) * P
                     w0 = (2 * q + u) * P
                     nc.tensor.transpose(bank[:, k0 : k0 + P], w_val[h][:].bitcast(F32)[:, w0 : w0 + P], ident[:])
-            if q % 2 == 0:
-                w_grp[q // 2] = two.tile([P, 8 * NB], BF16, name="w_grp", align_bytes=64)
+            w_grp[q] = three.tile([P, 4 * NB], BF16, name="w_grp", align_bytes=64)
 
             def copy_out():
-                words = w_grp[q // 2][:, q % 2 * 1024 : (q % 2 + 1) * 1024].bitcast(F32)
+                words = w_grp[q][:].bitcast(F32)
                 nc.scalar.copy(out=words.rearrange("p (n u) -> p n u", u=2), in_=bank[:].rearrange("p (u n) -> p n u", u=2))
                 give_bank(bank)
 
             return copy_out
 
         def scale_weights(q):
-            values = w_grp[q // 2][:, q % 2 * 1024 : (q % 2 + 1) * 1024].rearrange("p (n t) -> p n t", t=4)
-            nc.vector.tensor_tensor(
+            values = w_grp[q][:].rearrange("p (n t) -> p n t", t=4)
+            nc.gpsimd.tensor_tensor(
                 out=values,
                 in0=values,
                 in1=w_scale[:, q * 4 : (q + 1) * 4].unsqueeze(1).to_broadcast([P, NB, 4]),
                 op=MULT,
             )
 
-        def quantise_weights(pair):
-            cols = slice(pair * 2 * NB, (pair + 1) * 2 * NB)
-            nc.vector.quantize_mx(out=w_codes[:, cols].bitcast(FP8X4), scales=w_scales[:, cols], in_=w_grp[pair][:])
+        def quantise_weights(q):
+            cols = slice(q * NB, (q + 1) * NB)
+            nc.vector.quantize_mx(out=w_codes[:, cols].bitcast(FP8X4), scales=w_scales[:, cols], in_=w_grp[q][:])
 
         all_passes = (4, 5, 0, 1, 2, 3)
-        project_at = {max(GROUPS * it + PROJECT_LAG, it + FIRST_PROJECT): it for it in range(IT)}
-        w_turn_at = {W_FROM + 4 + 3 * q // 2: q for q in range(PASSES)}
 
-        load(0, 4)
+        def arranged_in(k):
+            return k - 1 if k <= CATCH_UP else k - 2
+
+        beside = {W_FIRST - 2: ("rel", 0)}
+        for q in range(PASSES):
+            beside[W_FIRST + 2 * q] = ("w", q)
+        for it in range(1, IT - 2):
+            beside[W_FIRST + 2 * (PASSES + it - 1)] = ("rel", it)
+        rel_round = {job[1]: arranged_in(k) for k, job in beside.items() if job[0] == "rel"}
+        rel_round[IT - 2] = STEPS - 2
+        w_turn_at = {arranged_in(k) - W_AHEAD: job[1] for k, job in beside.items() if job[0] == "w"}
+        sums_turn_at = {t - 1: it for it, t in rel_round.items()}
+        project_at = {t: it for it, t in enumerate(PROJECT_AT)}
+        left = list(range(len(PROJECT_AT), IT - 1))
+
+        narrow_at = {t: [] for t in range(STEPS)}
+        for s in range(1, STEPS - 1):
+            tiles = [a for a in range(RG) if summed_by(s, a) == NARROW]
+            split = on_vector(s + 1) >= RG - 1 and len(tiles) > 1 and SPLIT_FROM <= s < STEPS - 2
+            for a in tiles:
+                narrow_at[s + 1 + (split and 2 * a >= len(tiles))].append((s, a))
+        keep_at = {}
+        for it in range(IT - 1):
+            last = max(t for t in narrow_at for s, a in narrow_at[t] if s // GROUPS == it)
+            keep_at[max(last, GROUPS * it + 3) + 1] = it
+
+        def narrow_of_round(t):
+            return [(s, a, v, j) for v in range(2) for s, a in narrow_at[t] for j in range(4)]
+
+        def finish(job):
+            if job[0] == "w":
+                quantise_weights(job[1])
+            else:
+                quantise_supports(job[1], 4)
+
+        def arrange(k):
+            n = RG - on_vector(k)
+            if k < 2:
+                for a in range(n):
+                    cross(k, a, 1)
+                    nc.vector.memset(rep[RG * k + a][:], 0.0)
+            elif n == RG and k <= HALVED:
+                cross(k, 0, 2)
+                cross(k, 2, 2)
+            elif n:
+                cross(k, 0, n)
+            job = beside.get(k)
+            if job and job[0] == "w":
+                pick_values(w_scale, scale_masked, job[1], 1)
+            elif job:
+                collect_sums(job[1])
+            if k - 2 in beside:
+                finish(beside[k - 2])
+            if k == W_FIRST - 2:
+                mask_rows(scale_masked, scale_rows, F)
+            if job and job[0] == "w":
+                scale_weights(job[1])
+            elif job:
+                relation_part(job[1], nc.gpsimd)
+            for a in range(n, RG):
+                sort_and_sum(k, a)
+
         load_features()
-        for s in range(1, PREFETCH):
+        load(0, 4)
+        load(1, 4)
+        for s in range(2, PREFETCH):
             load(s, 2)
 
-        to_clear = [key for key in rep if key.count(NARROW) < R]
-        for key in to_clear[:3]:
-            nc.vector.memset(rep[key][:], 0.0)
+        cross_features(0)
+        cross_features(1)
         arrange(0)
-        for key in to_clear[3:]:
-            nc.vector.memset(rep[key][:], 0.0)
-        nc.vector.tensor_reduce(out=pick[:], in_=ident[:].rearrange("p (g x) -> p x g", x=GROUP), axis=AXIS_X, op=ADD)
         for s in range(STEPS - 1):
             it, phase = s // GROUPS - 1, s % GROUPS
-            w = s - W_FROM
             if s == 0:
                 load_rows(rel_rows, relation_features[0])
-            if w in (-3, -2):
-                nc.sync.dma_start(out=w_bytes[w + 3][:], in_=Wb_bytes[(w + 3) * P : (w + 4) * P, :])
-            if w == 0:
+            if s in W_LOAD:
+                h = W_LOAD.index(s)
+                nc.sync.dma_start(out=w_bytes[h][:], in_=Wb_bytes[h * P : (h + 1) * P, :])
+            if s == W_LOAD[1]:
                 load_rows(scale_rows, Wb_scale.rearrange("o (r f) -> (o r) f", f=F))
             if s + PREFETCH < STEPS:
                 load(s + PREFETCH, 2 if s + PREFETCH <= HALVED else 1)
 
             banks, later = [], []
-            if s > BAND_STEPS:
+            if s > BAND_UNTIL:
                 banks = [turn(s, a) for a in range(RG)]
+            by_vector = int(s in EMPTY_AT)
+            if by_vector:
+                empty(s, 0, banks[0], nc.vector.tensor_copy)
+
+            ahead = [k for k in range(1, STEPS) if arranged_in(k) == s]
+            early = s <= EARLY
+            if early:
+                arrange(ahead[0])
+            if s == 1:
+                quantise_features(1)
+            if s >= 1:
+                quantise(s - 1)
+            if s == 1:
+                interleave_features()
+                nc.vector.tensor_reduce(
+                    out=pick[:], in_=ident[:].rearrange("p (g x) -> p x g", x=GROUP), axis=AXIS_X, op=ADD
+                )
+                quantise_features(0)
+            if s == 3:
+                mask_rows(rel_masked, rel_rows, DR)
+            if s == 4:
+                pick_values(relf, rel_masked, 0, 2)
+            if it >= 1 and phase == 0:
+                quantise_supports(it - 1, 0, 4)
+            for k in ahead[early:]:
+                arrange(k)
+            for w in range(4):
+                if WIDEN_AT[w] == s:
+                    widen_weights(w // 2, w % 2)
+            if s == STEPS - 2:
+                collect_sums(IT - 2)
+                relation_part(IT - 2, nc.vector)
+
+            if s > BAND_UNTIL:
                 if it >= 0 and phase >= 2:
                     later.append(turn_supports(it, 2 * (phase - 2)))
                 if s == STEPS - 2:
                     later.append(turn_supports(it, 2))
                 if s in w_turn_at:
                     later.append(turn_weights(w_turn_at[s]))
-
-            on_vector = it >= 0 and phase == 2 and not has_window(s)
-            if on_vector:
-                collect_sums(it)
-            ahead = s + 2 if s > CATCH_UP else s + 1
-            by_vector = range(RG - vector_empties(s), RG)
-            if has_window(s):
-                collect_sums(it)
-                relation_part(it, nc.gpsimd)
-                sum_tiles(ahead)
-                for a in by_vector:
-                    empty(s, a, banks[a], nc.vector.tensor_copy)
-                cross_tiles(ahead)
-            elif 2 <= s <= CATCH_UP:
-                arrange(s + 1)
-            if s >= 1:
-                quantise(s - 1)
-            if not has_window(s):
-                for a in by_vector:
-                    empty(s, a, banks[a], nc.vector.tensor_copy)
-            if s - 1 in w_turn_at:
-                scale_weights(w_turn_at[s - 1])
-            if s == 0:
-                interleave_features()
-            if s < 2:
-                arrange(s + 1)
-            if s == 0:
-                quantise_features(0)
-            if s == 1:
-                quantise_features(1)
-            if s == ROWS_AT:
-                mask_rows(rel_masked, rel_rows, DR)
-            if s == ROWS_AT + 1:
-                pick_values(relf, rel_masked)
-            if w == 3:
-                mask_rows(scale_masked, scale_rows, F)
-            if w == 4:
-                pick_values(w_scale, scale_masked)
-            if 0 <= w < 4:
-                widen_weights(w // 2, w % 2)
-            if s == CATCH_UP or (CATCH_UP < s < STEPS - 2 and not has_window(s)):
-                arrange(s + 2)
-            if on_vector:
-                relation_part(it, nc.vector)
-            if w_turn_at.get(s - 2, 0) % 2:
-                quantise_weights(w_turn_at[s - 2] // 2)
-            if it >= 0 and phase == 3:
-                quantise_supports(it, 4)
-            if it >= 1 and phase == 0:
-                quantise_supports(it - 1, 0, 4)
-
-            if it >= 0 and phase == 1:
-                keep_sums(it)
-                spread_sums(it)
-            if s <= BAND_STEPS:
+            if s in keep_at:
+                keep_sums(keep_at[s])
+                spread_sums(keep_at[s])
+            narrow = narrow_of_round(s)
+            if s <= BAND_UNTIL:
                 for a in range(RG):
                     bank = turn(s, a)
                     empty(s, a, bank)
                     give_bank(bank)
-                    if s == 0 and a >= 2:
-                        cross_features(a - 2)
-                    k = RG * s + a - BAND_LAG
-                    if 0 <= k < BAND_STEPS * RG and k % RG < 2:
-                        band_sum(k // RG, k % RG)
+                    k = RG * s + a
+                    if k in BAND_AT:
+                        band_sum(0, BAND_AT.index(k))
             else:
-                for a in range(RG - vector_empties(s)):
+                for a in range(by_vector, RG):
                     empty(s, a, banks[a])
                     give_bank(banks[a])
-            for copy_out in later:
-                copy_out()
-            for a in by_vector:
-                give_bank(banks[a])
-            narrow = narrow_sums(s - 1) if s >= 1 else []
-            short = s not in project_at
-            issue(narrow, EDGE if short else len(narrow) // 2)
+                    if a == by_vector + 1 and by_vector:
+                        give_bank(banks[0])
+                for copy_out in later:
+                    copy_out()
             if s >= 2:
-                aggregate(s - 2, between=narrow if short else None)
+                issue(narrow, EDGE if s not in keep_at else 0)
+                aggregate_half(s - 2, 0)
+                issue(narrow, len(narrow) - EDGE)
+                aggregate_half(s - 2, 1)
                 keep_supports(s - 2)
             if s in project_at:
                 project(project_at[s], all_passes, 4, 3)
                 store(project_at[s])
             issue(narrow, len(narrow))
-            if it >= 0 and phase == 1:
-                turn_sums(it)
+            if s in sums_turn_at:
+                turn_sums(sums_turn_at[s])
 
         s, it = STEPS - 1, IT - 1
         quantise(s - 1)
@@ -637,7 +651,7 @@ def tile_relationalgraphconvolution_pa_kernel(
             bank = turn(s, a)
             empty(s, a, bank, nc.vector.tensor_copy if a == 3 else nc.scalar.copy)
             give_bank(bank)
-        narrow = narrow_sums(s - 1)
+        narrow = narrow_of_round(s)
         issue(narrow, EDGE)
         aggregate(s - 2)
         issue(narrow, len(narrow))
@@ -654,10 +668,12 @@ def tile_relationalgraphconvolution_pa_kernel(
             aggregate(s, a0, 2)
             keep_supports(s, a0, 2)
         relation_part(it, nc.vector)
-        project(it - 1, all_passes, 4, 3)
+        for k in left:
+            project(k, all_passes, 4, 3)
         for q in range(4):
             turn_supports(it, q, 1)()
-        store(it - 1)
+        for k in left:
+            store(k)
         quantise_supports(it, 0, 1)
         quantise_supports(it, 4)
         for q in range(1, 4):

@@ -28,23 +28,28 @@ HALVED = 7
 W_FIRST = 9
 W_AHEAD = 1
 WEAVE = 0
-W_LOAD = (0, 2)
-WIDEN_AT = (3, 3, 5, 5)
+W_LOAD = (0, 1)
+WIDEN_AT = (3, 3, 4, 4)
 FEATURES_FIRST = 1
-EARLY = 5
+EARLY = 4
 BAND_UNTIL = 2
 BAND_AT = (4, 7, 10, 11)
 CROSS_AT = (6, 7)
 CATCH_UP = 8
 SPREADS = 4
-MANY = 5
+MANY = 4
 BAND_STEPS = 1
 EXTRA_V = {}
-PROJECT_AT = (19, 21, 23, 25, 27, 29)
+PROJECT_AT = (19, 21, 23, 25, 27)
 SWAP = 1
+REL0_G = 0
+REL0_AT = 6
+DRAIN_V = (0, 2)
+LAST_V = (1,)
+COVER_FROM = 14
 SPLIT_FROM = 4
 PROJECT_EVERY = 2
-EMPTY_AT = range(W_FIRST - 1, W_FIRST + 2 * PASSES - 1, 2)
+SWAPPED = range(W_FIRST, W_FIRST + 2 * PASSES, 2)
 
 F32 = mybir.dt.float32
 BF16 = mybir.dt.bfloat16
@@ -64,15 +69,19 @@ def first_relation(s):
 
 
 def on_vector(s):
-    if s % 2 and s >= W_FIRST - 2:
-        return RG - (s - 1 in EMPTY_AT and SWAP)
+    if s == STEPS - 3:
+        return 0
+    if s % 2 and s >= W_FIRST - 2 * REL0_G:
+        return RG - (s in SWAPPED)
+    if s == STEPS - 2:
+        return RG
     return EXTRA_V.get(s, 0)
 
 
 def summed_by(s, a):
     if a >= RG - on_vector(s):
         return VECTOR
-    return BAND if s == 0 else NARROW
+    return BAND if s == 0 and a < len(BAND_AT) else NARROW
 
 
 def tile_relationalgraphconvolution_pa_kernel(
@@ -315,7 +324,7 @@ def tile_relationalgraphconvolution_pa_kernel(
 
         def turn_supports(it, q0, n=2, copy=nc.scalar.copy):
             if q0 == 0:
-                sgn[it] = two.tile([P, 2048], BF16, name="sgn", align_bytes=64)
+                sgn[it] = many.tile([P, 2048], BF16, name="sgn", align_bytes=64)
             bank = take_bank()
             for k in range(2 * n):
                 w0 = (2 * q0 + k) * P
@@ -404,7 +413,7 @@ def tile_relationalgraphconvolution_pa_kernel(
             give_bank(turned[it])
 
         def relation_part(it, engine):
-            sgr[it] = two.tile([P, 1024], BF16, name="sgr", align_bytes=64)
+            sgr[it] = three.tile([P, 1024], BF16, name="sgr", align_bytes=64)
             engine.tensor_tensor(
                 out=sgr[it][:].rearrange("p (b i t) -> p b i t", b=2, t=4),
                 in0=sums[it][:].unsqueeze(1).unsqueeze(3).to_broadcast([P, 2, P, 4]),
@@ -414,8 +423,8 @@ def tile_relationalgraphconvolution_pa_kernel(
 
         def quantise_supports(it, q0, n=2):
             if it not in scodes:
-                scodes[it] = many.tile([P, PASSES * P], U32, name="scodes", align_bytes=64)
-                sscales[it] = many.tile([P, PASSES * P], U8, name="sscales", align_bytes=64)
+                scodes[it] = three.tile([P, PASSES * P], U32, name="scodes", align_bytes=64)
+                sscales[it] = three.tile([P, PASSES * P], U8, name="sscales", align_bytes=64)
             cols = slice(q0 * P, (q0 + n) * P)
             nc.vector.quantize_mx(
                 out=scodes[it][:, cols].bitcast(FP8X4),
@@ -485,28 +494,30 @@ def tile_relationalgraphconvolution_pa_kernel(
         all_passes = (4, 5, 0, 1, 2, 3)
 
         def arranged_in(k):
-            return k - 1 if k <= CATCH_UP else k - 2
+            return k - 1 if k <= CATCH_UP else k - 2 - (k == STEPS - 2)
 
-        beside = {W_FIRST - 2: ("rel", 0)}
+        beside = {W_FIRST - 2: ("rel", 0)} if REL0_G else {}
         for q in range(PASSES):
             beside[W_FIRST + 2 * q] = ("w", q)
-        for it in range(1, IT - 2):
-            beside[W_FIRST + 2 * (PASSES + it - 1)] = ("rel", it)
+        for it in range(1, IT - 1):
+            beside[W_FIRST + 2 * (PASSES + it - 1) + (it == IT - 3)] = ("rel", it)
         rel_round = {job[1]: arranged_in(k) for k, job in beside.items() if job[0] == "rel"}
-        rel_round[IT - 2] = STEPS - 2
+        if not REL0_G:
+            rel_round[0] = REL0_AT
         w_turn_at = {arranged_in(k) - W_AHEAD: job[1] for k, job in beside.items() if job[0] == "w"}
         sums_turn_at = {t - 1: it for it, t in rel_round.items()}
         project_at = {t: it for it, t in enumerate(PROJECT_AT)}
+        node_at = {max(t - 1, GROUPS * it + 8): it for it, t in enumerate(PROJECT_AT + (29,))}
         left = list(range(len(PROJECT_AT), IT - 1))
 
         narrow_at = {t: [] for t in range(STEPS)}
-        for s in range(1, STEPS - 1):
+        for s in range(STEPS - 1):
             tiles = [a for a in range(RG) if summed_by(s, a) == NARROW]
-            split = on_vector(s + 1) >= RG - 1 and len(tiles) > 1 and SPLIT_FROM <= s < STEPS - 2
+            split = on_vector(s + 1) >= RG - 1 and len(tiles) > 1 and SPLIT_FROM <= s < STEPS - 6
             for a in tiles:
                 narrow_at[s + 1 + (split and 2 * a >= len(tiles))].append((s, a))
         keep_at = {}
-        for it in range(IT - 1):
+        for it in range(IT):
             last = max(t for t in narrow_at for s, a in narrow_at[t] if s // GROUPS == it)
             keep_at[max(last, GROUPS * it + 3) + 1] = it
 
@@ -519,32 +530,51 @@ def tile_relationalgraphconvolution_pa_kernel(
             else:
                 quantise_supports(job[1], 4)
 
-        def arrange(k):
+        def cross_step(k):
             n = RG - on_vector(k)
-            if k < 2:
-                for a in range(n):
-                    cross(k, a, 1)
-                    nc.vector.memset(rep[RG * k + a][:], 0.0)
-            elif n == RG and k <= HALVED:
+            if n == RG and k <= HALVED:
                 cross(k, 0, 2)
                 cross(k, 2, 2)
             elif n:
                 cross(k, 0, n)
+
+        def arrange(k):
+            n = RG - on_vector(k)
+            if k < 2:
+                for a in range(RG):
+                    if a < n:
+                        cross(k, a, 1)
+                    else:
+                        sort_and_sum(k, a)
+                    nc.vector.memset(rep[RG * k + a][:], 0.0)
+                return
             job = beside.get(k)
+            if k == CATCH_UP + 1:
+                cross_step(k - 1)
+            cross_step(k)
             if job and job[0] == "w":
                 pick_values(w_scale, scale_masked, job[1], 1)
             elif job:
                 collect_sums(job[1])
-            if k - 2 in beside:
-                finish(beside[k - 2])
-            if k == W_FIRST - 2:
-                mask_rows(scale_masked, scale_rows, F)
+            earlier = [j for j in beside if j < k]
+            if job and earlier:
+                finish(beside[max(earlier)])
+            for j in covers.get(k, ()):
+                cross_step(j)
+            if k == W_FIRST:
+                relation_part(0, nc.vector)
+            if k == W_FIRST + 2:
+                quantise_supports(0, 4)
             if job and job[0] == "w":
                 scale_weights(job[1])
             elif job:
                 relation_part(job[1], nc.gpsimd)
             for a in range(n, RG):
                 sort_and_sum(k, a)
+
+        covers = {k: (k + 1,) for k in beside if COVER_FROM <= k + 1 < STEPS - 2}
+        covers[STEPS - 2] = (STEPS - 3,)
+        covered = [CATCH_UP] + [j for k in covers for j in covers[k]]
 
         load_features()
         load(0, 4)
@@ -555,7 +585,7 @@ def tile_relationalgraphconvolution_pa_kernel(
         cross_features(0)
         cross_features(1)
         arrange(0)
-        for s in range(STEPS - 1):
+        for s in range(STEPS - 2):
             it, phase = s // GROUPS - 1, s % GROUPS
             if s == 0:
                 load_rows(rel_rows, relation_features[0])
@@ -570,11 +600,11 @@ def tile_relationalgraphconvolution_pa_kernel(
             banks, later = [], []
             if s > BAND_UNTIL:
                 banks = [turn(s, a) for a in range(RG)]
-            by_vector = int(s in EMPTY_AT)
+            by_vector = int(s in [arranged_in(k) + 1 for k in SWAPPED])
             if by_vector:
                 empty(s, 0, banks[0], nc.vector.tensor_copy)
 
-            ahead = [k for k in range(1, STEPS) if arranged_in(k) == s]
+            ahead = [k for k in range(1, STEPS) if arranged_in(k) == s and k not in covered]
             early = s <= EARLY
             if early:
                 arrange(ahead[0])
@@ -592,22 +622,20 @@ def tile_relationalgraphconvolution_pa_kernel(
                 mask_rows(rel_masked, rel_rows, DR)
             if s == 4:
                 pick_values(relf, rel_masked, 0, 2)
-            if it >= 1 and phase == 0:
-                quantise_supports(it - 1, 0, 4)
+            if s == REL0_AT and not REL0_G:
+                collect_sums(0)
+                mask_rows(scale_masked, scale_rows, F)
+            if s in node_at:
+                quantise_supports(node_at[s], 0, 4)
             for k in ahead[early:]:
                 arrange(k)
             for w in range(4):
                 if WIDEN_AT[w] == s:
                     widen_weights(w // 2, w % 2)
-            if s == STEPS - 2:
-                collect_sums(IT - 2)
-                relation_part(IT - 2, nc.vector)
 
             if s > BAND_UNTIL:
                 if it >= 0 and phase >= 2:
                     later.append(turn_supports(it, 2 * (phase - 2)))
-                if s == STEPS - 2:
-                    later.append(turn_supports(it, 2))
                 if s in w_turn_at:
                     later.append(turn_weights(w_turn_at[s]))
             if s in keep_at:
@@ -643,40 +671,54 @@ def tile_relationalgraphconvolution_pa_kernel(
             if s in sums_turn_at:
                 turn_sums(sums_turn_at[s])
 
-        s, it = STEPS - 1, IT - 1
+        s, it = STEPS - 2, IT - 1
+        banks = [turn(s, a) for a in range(RG)]
+        later = [turn_supports(it - 1, 0)]
         quantise(s - 1)
-        quantise_supports(it - 1, 0, 4)
         quantise_supports(it - 1, 4)
         for a in range(RG):
-            bank = turn(s, a)
-            empty(s, a, bank, nc.vector.tensor_copy if a == 3 else nc.scalar.copy)
-            give_bank(bank)
+            empty(s, a, banks[a])
+            give_bank(banks[a])
         narrow = narrow_of_round(s)
-        issue(narrow, EDGE)
+        issue(narrow, len(narrow) // 2)
         aggregate(s - 2)
         issue(narrow, len(narrow))
+        later.append(turn_supports(it - 1, 2))
+        later[0]()
         keep_supports(s - 2)
         keep_sums(it)
         spread_sums(it)
-        aggregate(s - 1)
-        keep_supports(s - 1)
+        s = STEPS - 1
+        banks = [turn(s, a) for a in range(2)]
+        later[1]()
+        banks.extend(turn(s, a) for a in range(2, RG))
         turn_sums(it)
+        quantise(s - 1)
+        aggregate(s - 2)
+        for a in range(RG):
+            empty(s, a, banks[a], nc.vector.tensor_copy if a in DRAIN_V else nc.scalar.copy)
+            give_bank(banks[a])
+        collect_sums(it)
+        aggregate(s - 1)
+        keep_supports(s - 2)
+        for k in left[:-1]:
+            project(k, all_passes, 4, 3)
         quantise(s, 0, 2)
         quantise(s, 2, 2)
-        collect_sums(it)
+        keep_supports(s - 1)
+        for k in left[:-1]:
+            store(k)
+        quantise_supports(it - 1, 0, 4)
+        relation_part(it, nc.vector)
+        quantise_supports(it, 4)
         for a0 in (0, 2):
             aggregate(s, a0, 2)
             keep_supports(s, a0, 2)
-        relation_part(it, nc.vector)
-        for k in left:
-            project(k, all_passes, 4, 3)
+        project(it - 1, all_passes, 4, 3)
         for q in range(4):
-            turn_supports(it, q, 1)()
-        for k in left:
-            store(k)
-        quantise_supports(it, 0, 1)
-        quantise_supports(it, 4)
-        for q in range(1, 4):
+            turn_supports(it, q, 1, nc.vector.tensor_copy if q in LAST_V else nc.scalar.copy)()
+        store(it - 1)
+        for q in range(4):
             quantise_supports(it, q, 1)
-        project(it, (0, 4, 5, 1, 2, 3), 0, 3)
+        project(it, all_passes, 4, 3)
         store(it)

@@ -24,7 +24,7 @@ LEAD = 128
 PITCH = LEAD + N
 PASSES = F // 32
 PREFETCH = 5
-HALVED = 7
+HALVED = 9
 W_FIRST = 9
 W_AHEAD = 1
 WEAVE = 0
@@ -44,12 +44,15 @@ PROJECT_AT = (19, 21, 23, 25, 27)
 SWAP = 1
 REL0_G = 0
 REL0_AT = 6
-DRAIN_V = (0, 2)
+DRAIN_V = (0,)
 LAST_V = (1,)
 COVER_FROM = 14
 SPLIT_FROM = 4
 PROJECT_EVERY = 2
 SWAPPED = range(W_FIRST, W_FIRST + 2 * PASSES, 2)
+SHORT = (9, 11, 13, 15, 17, 19, 21, 25)
+DEFER = 1
+WIDEN_S = ()
 
 F32 = mybir.dt.float32
 BF16 = mybir.dt.bfloat16
@@ -72,7 +75,7 @@ def on_vector(s):
     if s == STEPS - 3:
         return 0
     if s % 2 and s >= W_FIRST - 2 * REL0_G:
-        return RG - (s in SWAPPED)
+        return RG - (s in SHORT)
     if s == STEPS - 2:
         return RG
     return EXTRA_V.get(s, 0)
@@ -452,15 +455,14 @@ def tile_relationalgraphconvolution_pa_kernel(
             give_bank(obank[it])
             nc.sync.dma_start(out=out[0, it * P : (it + 1) * P, :], in_=res[:])
 
-        def widen_weights(h, half):
+        def widen_weights(h, half, on_scalar):
             r0 = half * R // 2
-            nc.vector.tensor_scalar(
-                out=w_val[h][:].rearrange("p (m r f) -> p r m f", r=R, f=RUN)[:, r0 : r0 + R // 2],
-                in0=w_bytes[h][:, r0 * F : (r0 + R // 2) * F].bitcast(FP8),
-                scalar1=one[:],
-                scalar2=None,
-                op0=MULT,
-            )
+            dst = w_val[h][:].rearrange("p (m r f) -> p r m f", r=R, f=RUN)[:, r0 : r0 + R // 2]
+            src = w_bytes[h][:, r0 * F : (r0 + R // 2) * F].bitcast(FP8)
+            if on_scalar:
+                nc.scalar.copy(out=dst, in_=src)
+            else:
+                nc.vector.tensor_scalar(out=dst, in0=src, scalar1=one[:], scalar2=None, op0=MULT)
 
         def turn_weights(q):
             bank = take_bank()
@@ -507,7 +509,7 @@ def tile_relationalgraphconvolution_pa_kernel(
         w_turn_at = {arranged_in(k) - W_AHEAD: job[1] for k, job in beside.items() if job[0] == "w"}
         sums_turn_at = {t - 1: it for it, t in rel_round.items()}
         project_at = {t: it for it, t in enumerate(PROJECT_AT)}
-        node_at = {max(t - 1, GROUPS * it + 8): it for it, t in enumerate(PROJECT_AT + (29,))}
+        node_at = {max((t - 1) * DEFER, GROUPS * it + 8): it for it, t in enumerate(PROJECT_AT + (29,))}
         left = list(range(len(PROJECT_AT), IT - 1))
 
         narrow_at = {t: [] for t in range(STEPS)}
@@ -546,7 +548,7 @@ def tile_relationalgraphconvolution_pa_kernel(
                         cross(k, a, 1)
                     else:
                         sort_and_sum(k, a)
-                    nc.vector.memset(rep[RG * k + a][:], 0.0)
+                    chores[RG * k + a]()
                 return
             job = beside.get(k)
             if k == CATCH_UP + 1:
@@ -575,6 +577,17 @@ def tile_relationalgraphconvolution_pa_kernel(
         covers = {k: (k + 1,) for k in beside if COVER_FROM <= k + 1 < STEPS - 2}
         covers[STEPS - 2] = (STEPS - 3,)
         covered = [CATCH_UP] + [j for k in covers for j in covers[k]]
+
+        def clear(it):
+            return lambda: nc.vector.memset(rep[it][:], 0.0)
+
+        def make_pick():
+            nc.vector.tensor_reduce(
+                out=pick[:], in_=ident[:].rearrange("p (g x) -> p x g", x=GROUP), axis=AXIS_X, op=ADD
+            )
+
+        chores = [interleave_features, make_pick, lambda: quantise_features(0), clear(0)]
+        chores.extend([clear(1), lambda: quantise_features(1), clear(2), lambda: None])
 
         load_features()
         load(0, 4)
@@ -609,15 +622,10 @@ def tile_relationalgraphconvolution_pa_kernel(
             if early:
                 arrange(ahead[0])
             if s == 1:
-                quantise_features(1)
+                for tile in rep[3:]:
+                    nc.vector.memset(tile[:], 0.0)
             if s >= 1:
                 quantise(s - 1)
-            if s == 1:
-                interleave_features()
-                nc.vector.tensor_reduce(
-                    out=pick[:], in_=ident[:].rearrange("p (g x) -> p x g", x=GROUP), axis=AXIS_X, op=ADD
-                )
-                quantise_features(0)
             if s == 3:
                 mask_rows(rel_masked, rel_rows, DR)
             if s == 4:
@@ -630,8 +638,8 @@ def tile_relationalgraphconvolution_pa_kernel(
             for k in ahead[early:]:
                 arrange(k)
             for w in range(4):
-                if WIDEN_AT[w] == s:
-                    widen_weights(w // 2, w % 2)
+                if WIDEN_AT[w] == s and w not in WIDEN_S:
+                    widen_weights(w // 2, w % 2, False)
 
             if s > BAND_UNTIL:
                 if it >= 0 and phase >= 2:
@@ -658,6 +666,9 @@ def tile_relationalgraphconvolution_pa_kernel(
                         give_bank(banks[0])
                 for copy_out in later:
                     copy_out()
+            for w in WIDEN_S:
+                if WIDEN_AT[w] == s:
+                    widen_weights(w // 2, w % 2, True)
             if s >= 2:
                 issue(narrow, EDGE if s not in keep_at else 0)
                 aggregate_half(s - 2, 0)

@@ -21,38 +21,55 @@ BANKS = 8
 EDGE = 4
 NARROW, BAND, VECTOR = range(3)
 LEAD = 128
-PITCH = LEAD + N
 PASSES = F // 32
 PREFETCH = 5
+RAWS = 8
+PAIRED = 1
 HALVED = 9
-W_FIRST = 9
-W_AHEAD = 1
-WEAVE = 0
-W_LOAD = (0, 1)
-WIDEN_AT = (3, 3, 4, 4)
-FEATURES_FIRST = 1
+FIRST_WINDOW = 7
+W_BEHIND = (4, 4)
+ROWS_BEHIND = 2
+WIDEN_AT = (4, 4, 5, 5, 5, 5, 6, 6, 7, 7)
+W_ORDER = (0, 1, 2, 3, 4, 5)
+CONST_AT = 4
 EARLY = 4
 BAND_UNTIL = 2
-BAND_AT = (4, 7, 10, 11)
-CROSS_AT = (6, 7)
+BAND_AT = ()
 CATCH_UP = 8
-SPREADS = 4
-MANY = 4
-BAND_STEPS = 1
-EXTRA_V = {}
-PROJECT_AT = (19, 21, 23, 25, 27)
-SWAP = 1
-REL0_G = 0
-REL0_AT = 6
-DRAIN_V = (0,)
-LAST_V = (1,)
+EXTRA_V = {3: 1}
+PROJECT_AT = (20, 22, 24, 26, 28)
 COVER_FROM = 14
 SPLIT_FROM = 4
-PROJECT_EVERY = 2
-SWAPPED = range(W_FIRST, W_FIRST + 2 * PASSES, 2)
-SHORT = (9, 11, 13, 15, 17, 19, 21, 25)
-DEFER = 1
-WIDEN_S = ()
+SHORT = (13, 15, 17)
+SWAPPED = (12, 14, 16)
+W_EXIT_V = ()
+W_EARLY = 0
+JOBS = "w3 w4 w5 r0 r1 r2 r3 r4 r5 r6"
+RC = 4
+NC = 10
+SUMS_LATE = 0
+WINDOWS = (13, 15, 17, 19, 21, 23, 25, 27, 30, 31)
+FUSED_AT = {6: 0, 8: 1, 10: 2}
+PAIR_AT = (5, 7, 9, 11)
+W_TURN = {}
+FIRSTP = "40"
+DRAIN = "t0 t1 t2 t3 S7 q30 a29 e0 e1 e2 E3 a30 k29 h0 h1 p5.45 A0 k30 x14.0.2 A1 K0 K1 y14.0 C7 u12.0.2 r6 u13.0.2 p5.0123 R7 x15.0.2 y15.0 z5 p6.450123 u14.0.2 r7 u15.0.2 z6 p7.024513 z7"
+PAIR_LAG = 4
+VX = {}
+OWN = ()
+HEAD = "f0 f1 x0.0 il x0.1 t0.0 t0.1 q@0 x0.2 t0.2 c0 x0.3 t0.3 c1 q@1 c2 x1.0 x1.1 b0.0 t1.0 t1.1 h0.0 n0.1 b0.2 x1.2 x1.3 c3 t1.2 t1.3 h0.1 x2.0 x2.1 n0.3 b1.0 t2.0 t2.1 a0 cf h1.0 x2.2 x2.3 n1.1 t2.2 t2.3 k0 b1.2 h1.1 sf x3.0 x3.1 h2.0 n1.3 t3.0 t3.1 a1 x3.2 s3.3 cb n2.0 n2.1 t3.2 t3.3 k1 n2.2 n2.3 h2.1 x4.0 x4.1 c4 c5 x4.2 x4.3 c6 c7"
+HEAD_ROUNDS = 4
+VH = {4: "w0 q3 w1 x5.0 x5.1 w2 x5.2 x5.3", 5: "q4 w3 w4 X6 w5", 6: "F0 q5 X7 w6 Q0", 7: "X8 q6 u0 w7 X9", 8: "F1 q7 X10 w8 Q1", 9: "q8 X11 u1 w9", 10: "F2 q9 X12 Q2"}
+FACTORS_AT = 4
+SINGLY = 1
+Q_FIRST = 1
+KEEP_LEAD = 0
+DRAIN_V = (0,)
+LAST_V = 0
+UNIT_LAG = 4
+QLAG = 1
+SGN = 3
+CLEAR_AT = 1
 
 F32 = mybir.dt.float32
 BF16 = mybir.dt.bfloat16
@@ -67,24 +84,36 @@ AXIS_X = mybir.AxisListType.X
 FLOPS = 2 * (R * N * N * DE + N * R * F * NB)
 
 
-def first_relation(s):
-    return GROUP_AT[s % GROUPS] * RG
+def paired(s):
+    return s < 2 * GROUPS * PAIRED
+
+
+def tile_of(s, a):
+    if paired(s):
+        return a % 2, (2 * s + a // 2 - RG) % R
+    return s // GROUPS, GROUP_AT[s % GROUPS] * RG + a
+
+
+def row_start(s, a):
+    if paired(s):
+        return LEAD + a // 2 * (LEAD + 2 * N) + a % 2 * N
+    return LEAD + a * (LEAD + N)
 
 
 def on_vector(s):
-    if s == STEPS - 3:
-        return 0
-    if s % 2 and s >= W_FIRST - 2 * REL0_G:
+    if s in WINDOWS:
         return RG - (s in SHORT)
-    if s == STEPS - 2:
-        return RG
     return EXTRA_V.get(s, 0)
+
+
+def band_tiles():
+    return [(s, a) for s in range(2) for a in range(RG) if tile_of(s, a)[0] == 0]
 
 
 def summed_by(s, a):
     if a >= RG - on_vector(s):
         return VECTOR
-    return BAND if s == 0 and a < len(BAND_AT) else NARROW
+    return BAND if (s, a) in band_tiles() else NARROW
 
 
 def tile_relationalgraphconvolution_pa_kernel(
@@ -93,27 +122,33 @@ def tile_relationalgraphconvolution_pa_kernel(
     nc = tc.nc
     with ExitStack() as ctx:
         keep = ctx.enter_context(tc.tile_pool(name="keep", bufs=1))
-        rawp = ctx.enter_context(tc.tile_pool(name="rawp", bufs=PREFETCH + 3))
+        rawp = ctx.enter_context(tc.tile_pool(name="rawp", bufs=RAWS))
         onep = ctx.enter_context(tc.tile_pool(name="onep", bufs=8))
         two = ctx.enter_context(tc.tile_pool(name="two", bufs=2))
         three = ctx.enter_context(tc.tile_pool(name="three", bufs=3))
-        many = ctx.enter_context(tc.tile_pool(name="many", bufs=MANY))
+        four = ctx.enter_context(tc.tile_pool(name="four", bufs=4))
+        rcp = ctx.enter_context(tc.tile_pool(name="rcp", bufs=RC))
+        ncp = ctx.enter_context(tc.tile_pool(name="ncp", bufs=NC))
+        sgnp = ctx.enter_context(tc.tile_pool(name="sgnp", bufs=SGN))
         psum = ctx.enter_context(tc.psum_pool(name="psum", bufs=1))
         ctx.enter_context(tc.manual_schedule())
 
         ident = keep.tile([P, P], F32, name="ident", align_bytes=64)
         make_identity(nc, ident[:])
         rs = keep.tile([P, STEPS * RG], F32, name="rs", align_bytes=64)
-        kinds = [[summed_by(GROUPS * it + GROUP_AT.index(r // RG), r % RG) for r in range(R)] for it in range(IT)]
+        place = {tile_of(s, a): (s, a) for s in range(STEPS) for a in range(RG)}
+        kinds = [[summed_by(*place[it, r]) for r in range(R)] for it in range(IT)]
         rep = [keep.tile([P, 3 * P], F32, name="rep%d" % it, align_bytes=64) for it in range(IT)]
         ones = keep.tile([P, GROUP], BF16, name="ones", align_bytes=64)
         nc.vector.memset(ones[:], 1.0)
         band = keep.tile([P, 2 * P - GROUP], BF16, name="band", align_bytes=64)
         nc.vector.memset(band[:], 0.0)
         nc.vector.memset(band[:, P - GROUP : P], 1.0)
-        pick = keep.tile([P, GROUP], F32, name="pick", align_bytes=64)
         select = keep.tile([P, 4 * P], BF16, name="select", align_bytes=64)
         nc.vector.memset(select[:], 0.0)
+        one = keep.tile([P, 1], F32, name="one", align_bytes=64)
+        nc.vector.memset(one[:], 1.0)
+        factor_cols = keep.tile([P, 4 * P], F32, name="factor_cols", align_bytes=64)
         for par in range(2):
             nc.vector.tensor_copy(
                 out=select[:].rearrange("p (c a j b x) -> p c a j b x", c=2, a=2, b=2, x=GROUP)[:, :, par, :, par, :],
@@ -123,18 +158,19 @@ def tile_relationalgraphconvolution_pa_kernel(
         nf_grp = keep.tile([P, 4 * 4 * DE], BF16, name="nf_grp", align_bytes=64)
         nf_codes = keep.tile([P, 4 * DE], U32, name="nf_codes", align_bytes=64)
         nf_scales = keep.tile([P, 4 * DE], U8, name="nf_scales", align_bytes=64)
-        rel_rows = keep.tile([P, DR], BF16, name="rel_rows", align_bytes=64)
-        rel_masked = keep.tile([P, DR], F32, name="rel_masked", align_bytes=64)
-        scale_rows = keep.tile([P, F], F32, name="scale_rows", align_bytes=64)
-        scale_masked = keep.tile([P, F], F32, name="scale_masked", align_bytes=64)
+        factor_rows = keep.tile([P, RG * F], F32, name="factor_rows", align_bytes=64)
+        node_rows = factor_rows[0:GROUPS, :]
+        rel_rows = factor_rows[32:34, 0 : R * 32]
+        relf_rows = factor_rows[64:66, :].bitcast(BF16)[:, 0 : R * 32]
         w_scale = keep.tile([P, PASSES * 4], F32, name="w_scale", align_bytes=64)
-        one = keep.tile([P, 1], F32, name="one", align_bytes=64)
-        nc.vector.memset(one[:], 1.0)
         relf = keep.tile([P, 2 * 4], F32, name="relf", align_bytes=64)
+        factors = keep.tile([P, PASSES * 4], F32, name="factors", align_bytes=64)
         w_bytes = [keep.tile([P, R * F], U8, name="w_bytes%d" % h, align_bytes=64) for h in range(2)]
         w_val = [keep.tile([P, R * F], BF16, name="w_val%d" % h, align_bytes=64) for h in range(2)]
         w_codes = keep.tile([P, PASSES * NB], U32, name="w_codes", align_bytes=64)
         w_scales = keep.tile([P, PASSES * NB], U8, name="w_scales", align_bytes=64)
+        n_codes = {}
+        n_scales = {}
 
         raw = {}
         window = {}
@@ -143,13 +179,19 @@ def tile_relationalgraphconvolution_pa_kernel(
         scales = {}
         mx = {}
         sums = {}
-        supn = {}
+        sup = {}
         sgn = {}
         sgr = {}
-        scodes = {}
-        sscales = {}
+        r_codes = {}
+        r_scales = {}
         obank = {}
         w_grp = {}
+        w_bank = {}
+
+        def couple_of(it, g):
+            if paired(GROUPS * it):
+                return (g + 1) % GROUPS, it
+            return 2 * it + GROUP_AT.index(g) // 2, GROUP_AT.index(g) % 2
 
         free_banks = list(range(BANKS - 2))
         held = {}
@@ -166,20 +208,33 @@ def tile_relationalgraphconvolution_pa_kernel(
         sums_bank = psum.tile([P, 512], F32, name="bank%d" % (BANKS - 1))
         first_sums = psum.tile([P, 512], F32, name="bank%d" % (BANKS - 2))
         held[BANKS - 2] = first_sums
-        turned = {0: first_sums}
+        turned = {}
 
-        def rows_of(s, a0, n, first):
-            return raw[s][:, first + a0 * PITCH : first + (a0 + n) * PITCH].rearrange("p (a q) -> p a q", q=PITCH)
+        def rows_of(s, a0, n, shift):
+            pitch = LEAD + (2 * N if paired(s) else N)
+            first = row_start(s, a0) + shift
+            return raw[s][:, first : first + n * pitch].rearrange("p (a q) -> p a q", q=pitch)
 
         def load(s, pieces=1):
-            it = s // GROUPS
-            raw[s] = rawp.tile([P, LEAD + RG * PITCH], BF16, name="raw", align_bytes=256)
+            raw[s] = rawp.tile([P, LEAD + RG * (LEAD + N)], BF16, name="raw", align_bytes=256)
+            it, r0 = tile_of(s, 0)
+            if paired(s):
+                rows = adj[0, r0 : r0 + 2, it * P : (it + 2) * P, :].rearrange("r (i h) j -> i r (h j)", h=2)
+                if pieces == 4:
+                    for a in range(RG):
+                        nc.sync.dma_start(
+                            out=raw[s][:, row_start(s, a) : row_start(s, a) + N], in_=rows[:, a // 2, a % 2 * N : (a % 2 + 1) * N]
+                        )
+                    return
+                n = 2 // pieces
+                for a0 in range(0, 2, n):
+                    nc.sync.dma_start(out=rows_of(s, 2 * a0, n, 0)[:, :, 0 : 2 * N], in_=rows[:, a0 : a0 + n])
+                return
             n = RG // pieces
             for a0 in range(0, RG, n):
-                r0 = first_relation(s) + a0
                 nc.sync.dma_start(
-                    out=rows_of(s, a0, n, LEAD)[:, :, 0:N],
-                    in_=adj[0, r0 : r0 + n, it * P : (it + 1) * P, :].rearrange("r i j -> i r j"),
+                    out=rows_of(s, a0, n, 0)[:, :, 0:N],
+                    in_=adj[0, r0 + a0 : r0 + a0 + n, it * P : (it + 1) * P, :].rearrange("r i j -> i r j"),
                 )
 
         def load_features():
@@ -220,46 +275,74 @@ def tile_relationalgraphconvolution_pa_kernel(
                 in_=nf_grp[:, v * 1024 : (v + 1) * 1024],
             )
 
-        def load_rows(dst, rows):
-            nc.sync.dma_start(out=dst[:], in_=rows.partition_broadcast(GROUP).rearrange("x r f -> r x f"))
-
-        def mask_rows(masked, rows, width):
-            nc.vector.tensor_tensor(
-                out=masked[:].rearrange("p (m x e) -> p m x e", x=GROUP, e=2),
-                in0=rows[:].rearrange("p (m x e) -> p m x e", x=GROUP, e=2),
-                in1=pick[:].unsqueeze(1).unsqueeze(3).to_broadcast([P, width // RUN, GROUP, 2]),
-                op=MULT,
+        def load_factors():
+            nc.sync.dma_start(out=node_rows, in_=Wb_scale.rearrange("o (g k) -> (o g) k", g=GROUPS))
+            nc.sync.dma_start(
+                out=rel_rows.rearrange("p (r f) -> p r f", f=32),
+                in_=Wb_scale.rearrange("o (r m f) -> (o m) r f", r=R, f=32)[4:6],
+            )
+            nc.sync.dma_start(
+                out=relf_rows.rearrange("p (r f) -> p r f", f=32),
+                in_=relation_features[0].rearrange("r (b f) -> b r f", f=32),
             )
 
-        def pick_values(dst, masked, q0, n):
-            nc.vector.tensor_reduce(
-                out=dst[:, q0 * 4 : (q0 + n) * 4].rearrange("p (m e) -> p m e", e=2),
-                in_=masked[:, q0 * 32 : (q0 + n) * 32].rearrange("p (m x e) -> p m e x", x=GROUP, e=2),
-                axis=AXIS_X,
-                op=ADD,
-            )
+        def sort_factors():
+            src = node_rows.rearrange("p (a m x e) -> p e a m x", a=RG, x=GROUP, e=2)
+            for u in range(2):
+                nc.vector.tensor_copy(
+                    out=factor_cols[0:GROUPS, u * 2 * P : (u + 1) * 2 * P].rearrange("p (e a q x) -> p e a q x", e=2, a=RG, x=GROUP),
+                    in_=src[:, :, :, u:8:2, :],
+                )
+            for p0, rows in ((32, rel_rows), (64, relf_rows)):
+                nc.vector.tensor_copy(
+                    out=factor_cols[p0 : p0 + 2, :].rearrange("p (u e r x) -> p u e r x", u=2, e=2, x=GROUP),
+                    in_=rows.rearrange("p (r u x e) -> p u e r x", u=2, x=GROUP, e=2),
+                )
+
+        def turn_factors():
+            bank = take_bank()
+            for t in range(4):
+                nc.tensor.transpose(bank[:, t * P : (t + 1) * P], factor_cols[:, t * P : (t + 1) * P], ident[:])
+
+            def copy_out():
+                cols = bank[:].rearrange("p (t j) -> p j t", t=4)
+                for dst, j0, n in ((factors[:, 0:16], 0, 4), (factors[:, 16:24], 32, 2), (relf[:], 64, 2)):
+                    nc.scalar.copy(out=dst.rearrange("p (j t) -> p j t", t=4), in_=cols[:, j0 : j0 + n, :])
+                give_bank(bank)
+
+            return copy_out
 
         def cross(s, a0, n):
-            for a in range(a0, a0 + n):
+            mirrored = paired(s) and a0 % 2
+            for a in range(a0, a0 + 2 * n, 2) if paired(s) else range(a0, a0 + n):
                 for c in range(2):
-                    first = a * PITCH // 2 + c * P
-                    window[s, a, c] = ((raw[s], first + (LEAD + N // 2) // 2), (raw[s], first + (LEAD - RUN) // 2))
-            odd = rows_of(s, a0, n, LEAD)[:, :, 0:N].rearrange("p a (h j o f) -> p a j h o f", h=2, o=2, f=RUN)
-            free = rows_of(s, a0, n, LEAD - RUN)[:, :, 0 : N + 4 * RUN]
-            free = free.rearrange("p a (h j o f) -> p a j h o f", h=2, o=2, f=RUN)
-            dst, src = free[:, :, 0:16, :, 0, :], odd[:, :, :, ::-1, 1, :]
+                    first = row_start(s, a) // 2 + c * P
+                    starts = (0, N // 2 + RUN) if mirrored else (N // 2, -RUN)
+                    window[s, a, c] = [(raw[s], first + w // 2) for w in starts]
+            if mirrored:
+                runs = rows_of(s, a0, n, -N)[:, :, N : 2 * N]
+                free = rows_of(s, a0, n, -N)[:, :, N : 2 * N + 4 * RUN]
+            else:
+                runs = rows_of(s, a0, n, 0)[:, :, 0:N]
+                free = rows_of(s, a0, n, -RUN)[:, :, 0 : N + 4 * RUN]
+            runs, free = [v.rearrange("p a (h j o f) -> p a j h o f", h=2, o=2, f=RUN) for v in (runs, free)]
+            if mirrored:
+                dst, src = free[:, :, 15::-1, ::-1, 0, :], runs[:, :, ::-1, :, 0, :]
+            else:
+                dst, src = free[:, :, 0:16, :, 0, :], runs[:, :, :, ::-1, 1, :]
             if n == 1:
                 dst, src = [v[:, 0].rearrange("p j h (k f) -> p k j h f", k=2) for v in (dst, src)]
             nc.vector.tensor_copy(out=dst, in_=src)
 
         def sort_and_sum(s, a):
-            k = s // GROUPS * R + first_relation(s) + a
+            it, r = tile_of(s, a)
+            k = it * R + r
             dst = onep.tile([P, N], BF16, name="sorted", align_bytes=64)
             for c in range(2):
                 window[s, a, c] = [(dst, (2 * u + c) * P) for u in range(2)]
             nc.vector.tensor_scalar(
                 out=dst[:].rearrange("p (u q f) -> p u q f", u=2, f=RUN),
-                in0=raw[s][:, LEAD + a * PITCH : LEAD + a * PITCH + N].rearrange("p (q u f) -> p u q f", u=2, f=RUN),
+                in0=raw[s][:, row_start(s, a) : row_start(s, a) + N].rearrange("p (q u f) -> p u q f", u=2, f=RUN),
                 scalar1=1.0,
                 scalar2=None,
                 op0=MULT,
@@ -302,11 +385,12 @@ def tile_relationalgraphconvolution_pa_kernel(
             if (s, a0) not in mx:
                 mx[s, a0] = take_bank()
             for a in tiles or range(a0, a0 + n):
+                slot = a % 2 * 2 + a // 2 if paired(s) else a - a0
                 for c in range(2):
                     cols = slice(a * 256 + c * P, a * 256 + (c + 1) * P)
                     f0 = (c + 2 * (summed_by(s, a) != VECTOR)) * DE
                     nc.tensor.matmul_mx(
-                        out=mx[s, a0][:, (a - a0) * DE : (a - a0 + 1) * DE],
+                        out=mx[s, a0][:, slot * DE : (slot + 1) * DE],
                         lhsT=codes[s][:, cols].bitcast(FP8X4),
                         lhsT_scale=scales[s][:, cols],
                         rhs=nf_codes[:, f0 : f0 + DE].bitcast(FP8X4),
@@ -316,26 +400,34 @@ def tile_relationalgraphconvolution_pa_kernel(
                     )
 
         def keep_supports(s, a0=0, n=RG):
-            it, r0 = s // GROUPS, first_relation(s) + a0
-            if r0 == 0:
-                supn[it] = two.tile([P, R * DE], BF16, name="supn", align_bytes=64)
-            nc.scalar.copy(
-                out=supn[it][:].rearrange("p (m r f) -> p m r f", r=R, f=RUN)[:, :, r0 : r0 + n, :],
-                in_=mx[s, a0][:, 0 : n * DE].rearrange("p (a m f) -> p m a f", a=n, f=RUN),
-            )
+            it, r0 = tile_of(s, a0)
+            k, w = couple_of(it, r0 // RG)
+            if k not in sup:
+                sup[k] = four.tile([P, 2 * RG * DE], BF16, name="sup", align_bytes=64)
+            dst = sup[k][:].rearrange("p (w u m f) -> p w u m f", w=2, u=2, f=RUN)
+            src = mx[s, a0][:, 0 : n * DE]
+            m0 = r0 % RG * 4
+            if paired(s):
+                nc.scalar.copy(
+                    out=dst[:, :, :, m0 : m0 + 8, :], in_=src.rearrange("p (w m u f) -> p w u m f", w=2, u=2, f=RUN)
+                )
+            else:
+                nc.scalar.copy(
+                    out=dst[:, w, :, m0 : m0 + 4 * n, :], in_=src.rearrange("p (m u f) -> p u m f", u=2, f=RUN)
+                )
             give_bank(mx[s, a0])
 
-        def turn_supports(it, q0, n=2, copy=nc.scalar.copy):
-            if q0 == 0:
-                sgn[it] = many.tile([P, 2048], BF16, name="sgn", align_bytes=64)
+        def turn_supports(k, w0=0, n=2, copy=nc.scalar.copy):
+            if w0 == 0:
+                sgn[k] = sgnp.tile([P, 1024], BF16, name="sgn", align_bytes=64)
             bank = take_bank()
-            for k in range(2 * n):
-                w0 = (2 * q0 + k) * P
-                nc.tensor.transpose(bank[:, k * P : (k + 1) * P], supn[it][:].bitcast(F32)[:, w0 : w0 + P], ident[:])
+            for j in range(2 * n):
+                c0 = (2 * w0 + j) * P
+                nc.tensor.transpose(bank[:, j * P : (j + 1) * P], sup[k][:].bitcast(F32)[:, c0 : c0 + P], ident[:])
 
             def copy_out():
                 copy(
-                    out=sgn[it][:, q0 * 512 : (q0 + n) * 512].bitcast(F32).rearrange("p (b i u) -> p b i u", b=n, u=2),
+                    out=sgn[k][:, w0 * 512 : (w0 + n) * 512].bitcast(F32).rearrange("p (b i u) -> p b i u", b=n, u=2),
                     in_=bank[:, 0 : n * 256].rearrange("p (b u i) -> p b i u", b=n, u=2),
                 )
                 give_bank(bank)
@@ -343,7 +435,8 @@ def tile_relationalgraphconvolution_pa_kernel(
             return copy_out
 
         def narrow_sum(s, a, v, j):
-            k0 = v * P + (first_relation(s) + a) * GROUP
+            it, r = tile_of(s, a)
+            k0 = it % 2 * 2 * P + v * P + r * GROUP
             c0 = a * N + j // 2 * 512 + v * 256
             nc.tensor.matmul(
                 sums_bank[:, k0 : k0 + GROUP],
@@ -363,16 +456,16 @@ def tile_relationalgraphconvolution_pa_kernel(
             return turned[it][:, 0 : 2 * P]
 
         def band_sum(s, a):
-            it, r = s // GROUPS, first_relation(s) + a
+            it, r = tile_of(s, a)
             for c in range(2):
                 words = grp[s][:, a * N + c * 512 : a * N + (c + 1) * 512].rearrange("p (i u e) -> p u i e", u=2, e=2)
                 for u in range(2):
                     nc.tensor.matmul(
-                        turned_sums(it).rearrange("p (i e) -> p i e", e=2),
+                        first_sums[:, 0 : 2 * P].rearrange("p (i e) -> p i e", e=2),
                         lhsT=band[:, P - GROUP * (r + 1) : 2 * P - GROUP * (r + 1)],
                         rhs=words[:, u],
                         start=(s == 0 and a == 0 and c == 0 and u == 0),
-                        stop=False,
+                        stop=((s, a) == band_tiles()[-1] and c == 1 and u == 1),
                     )
 
         def columns_of(it, kind):
@@ -382,7 +475,7 @@ def tile_relationalgraphconvolution_pa_kernel(
 
         def keep_sums(it):
             dst = rep[it][:, 0 : 2 * P].rearrange("p (v m) -> p v m", v=2)
-            src = sums_bank[:, 0 : 2 * P].rearrange("p (v m) -> p v m", v=2)
+            src = sums_bank[:, it % 2 * 2 * P : (it % 2 + 1) * 2 * P].rearrange("p (v m) -> p v m", v=2)
             for r0, r1 in columns_of(it, NARROW):
                 nc.scalar.copy(out=dst[:, :, r0 * GROUP : r1 * GROUP], in_=src[:, :, r0 * GROUP : r1 * GROUP])
 
@@ -396,22 +489,36 @@ def tile_relationalgraphconvolution_pa_kernel(
 
         def turn_sums(it):
             last = 2 if VECTOR in kinds[it] else 1
-            if it > 0:
-                turned[it] = take_bank()
+            turned[it] = take_bank()
             for v in range(last + 1):
                 nc.tensor.matmul(
                     turned_sums(it)[:, v * P : (v + 1) * P] if v < 2 else turned_sums(it)[:, 0 : 2 * P : 2],
                     lhsT=rep[it][:, v * P : (v + 1) * P],
                     rhs=ident[:],
-                    start=(v == 0 and it > 0),
+                    start=(v == 0),
                     stop=(v == last),
                     is_transpose=True,
                 )
 
-        def collect_sums(it):
-            sums[it] = two.tile([P, P], F32, name="sums", align_bytes=64)
+        def collect_band():
+            sums[0] = three.tile([P, P], F32, name="sums", align_bytes=64)
             nc.vector.tensor_reduce(
-                out=sums[it][:], in_=turned_sums(it).rearrange("p (i u) -> p i u", u=2), axis=AXIS_X, op=ADD
+                out=sums[0][96:P, :],
+                in_=first_sums[96:P, 0 : 2 * P].rearrange("p (i u) -> p i u", u=2),
+                axis=AXIS_X,
+                op=ADD,
+            )
+            give_bank(first_sums)
+
+        def collect_sums(it):
+            if it > 0:
+                sums[it] = three.tile([P, P], F32, name="sums", align_bytes=64)
+            p1 = P if it > 0 else 96
+            nc.vector.tensor_reduce(
+                out=sums[it][0:p1, :],
+                in_=turned_sums(it)[0:p1].rearrange("p (i u) -> p i u", u=2),
+                axis=AXIS_X,
+                op=ADD,
             )
             give_bank(turned[it])
 
@@ -424,25 +531,35 @@ def tile_relationalgraphconvolution_pa_kernel(
                 op=MULT,
             )
 
-        def quantise_supports(it, q0, n=2):
-            if it not in scodes:
-                scodes[it] = three.tile([P, PASSES * P], U32, name="scodes", align_bytes=64)
-                sscales[it] = three.tile([P, PASSES * P], U8, name="sscales", align_bytes=64)
-            cols = slice(q0 * P, (q0 + n) * P)
+        def quantise_couple(k, w0=0, n=2):
+            if k not in n_codes:
+                n_codes[k] = ncp.tile([P, 2 * P], U32, name="n_codes", align_bytes=64)
+                n_scales[k] = ncp.tile([P, 2 * P], U8, name="n_scales", align_bytes=64)
+            cols = slice(w0 * P, (w0 + n) * P)
             nc.vector.quantize_mx(
-                out=scodes[it][:, cols].bitcast(FP8X4),
-                scales=sscales[it][:, cols],
-                in_=sgr[it][:] if q0 == 4 else sgn[it][:, q0 * 512 : (q0 + n) * 512],
+                out=n_codes[k][:, cols].bitcast(FP8X4), scales=n_scales[k][:, cols], in_=sgn[k][:, w0 * 512 : (w0 + n) * 512]
             )
+
+        def quantise_relation_part(it):
+            r_codes[it] = rcp.tile([P, 2 * P], U32, name="r_codes", align_bytes=64)
+            r_scales[it] = rcp.tile([P, 2 * P], U8, name="r_scales", align_bytes=64)
+            nc.vector.quantize_mx(out=r_codes[it][:].bitcast(FP8X4), scales=r_scales[it][:], in_=sgr[it][:])
 
         def project(it, passes, first, last):
             for q in passes:
                 if q == first:
                     obank[it] = take_bank()
+                if q < GROUPS:
+                    k, w = couple_of(it, q)
+                    cols = slice(w * P, (w + 1) * P)
+                    words, exps = n_codes[k][:, cols], n_scales[k][:, cols]
+                else:
+                    cols = slice((q - GROUPS) * P, (q - GROUPS + 1) * P)
+                    words, exps = r_codes[it][:, cols], r_scales[it][:, cols]
                 nc.tensor.matmul_mx(
                     out=obank[it][:, 0:NB],
-                    lhsT=scodes[it][:, q * P : (q + 1) * P].bitcast(FP8X4),
-                    lhsT_scale=sscales[it][:, q * P : (q + 1) * P],
+                    lhsT=words.bitcast(FP8X4),
+                    lhsT_scale=exps,
                     rhs=w_codes[:, q * NB : (q + 1) * NB].bitcast(FP8X4),
                     rhs_scale=w_scales[:, q * NB : (q + 1) * NB],
                     start=(q == first),
@@ -453,32 +570,47 @@ def tile_relationalgraphconvolution_pa_kernel(
             res = three.tile([P, NB], F32, name="res", align_bytes=64)
             copy(out=res[:], in_=obank[it][:, 0:NB])
             give_bank(obank[it])
-            nc.sync.dma_start(out=out[0, it * P : (it + 1) * P, :], in_=res[:])
-
-        def widen_weights(h, half, on_scalar):
-            r0 = half * R // 2
-            dst = w_val[h][:].rearrange("p (m r f) -> p r m f", r=R, f=RUN)[:, r0 : r0 + R // 2]
-            src = w_bytes[h][:, r0 * F : (r0 + R // 2) * F].bitcast(FP8)
-            if on_scalar:
-                nc.scalar.copy(out=dst, in_=src)
+            if paired(GROUPS * it):
+                rows = out[0, it // 2 * 2 * P : (it // 2 + 1) * 2 * P, :].rearrange("(i h) n -> h i n", h=2)[it % 2]
             else:
-                nc.vector.tensor_scalar(out=dst, in0=src, scalar1=one[:], scalar2=None, op0=MULT)
+                rows = out[0, it * P : (it + 1) * P, :]
+            nc.sync.dma_start(out=rows, in_=res[:])
+
+        def widen_weights(h, g):
+            rows = w_bytes[h][:].rearrange("p (r k) -> p r k", k=F)
+            if g < GROUPS:
+                src = rows[:, g * RG : (g + 1) * RG, 0:DE]
+                dst = w_val[h][:, g * 512 : (g + 1) * 512].rearrange("p (u m f) -> p m u f", u=2, f=RUN)
+            else:
+                src = rows[:, :, DE:F]
+                dst = w_val[h][:, GROUPS * 512 :].rearrange("p (m r f) -> p r m f", r=R, f=RUN)
+            nc.vector.tensor_scalar(out=dst, in0=src.bitcast(FP8), scalar1=one[:], scalar2=None, op0=MULT)
 
         def turn_weights(q):
-            bank = take_bank()
+            w_bank[q] = take_bank()
             for u in range(2):
                 for h in range(2):
                     k0 = (u * 2 + h) * P
                     w0 = (2 * q + u) * P
-                    nc.tensor.transpose(bank[:, k0 : k0 + P], w_val[h][:].bitcast(F32)[:, w0 : w0 + P], ident[:])
+                    nc.tensor.transpose(w_bank[q][:, k0 : k0 + P], w_val[h][:].bitcast(F32)[:, w0 : w0 + P], ident[:])
+
+        def empty_weights(q, copy):
             w_grp[q] = three.tile([P, 4 * NB], BF16, name="w_grp", align_bytes=64)
+            copy(
+                out=w_grp[q][:].bitcast(F32).rearrange("p (n u) -> p n u", u=2),
+                in_=w_bank[q][:].rearrange("p (u n) -> p n u", u=2),
+            )
+            give_bank(w_bank[q])
 
-            def copy_out():
-                words = w_grp[q][:].bitcast(F32)
-                nc.scalar.copy(out=words.rearrange("p (n u) -> p n u", u=2), in_=bank[:].rearrange("p (u n) -> p n u", u=2))
-                give_bank(bank)
-
-            return copy_out
+        def empty_scaled(q):
+            w_grp[q] = three.tile([P, 4 * NB], BF16, name="w_grp", align_bytes=64)
+            nc.vector.tensor_tensor(
+                out=w_grp[q][:].rearrange("p (n u e) -> p n u e", u=2, e=2),
+                in0=w_bank[q][:].bitcast(BF16).rearrange("p (u n e) -> p n u e", u=2, e=2),
+                in1=factors[:, q * 4 : (q + 1) * 4].rearrange("p (u e) -> p u e", u=2).unsqueeze(1).to_broadcast([P, NB, 2, 2]),
+                op=MULT,
+            )
+            give_bank(w_bank[q])
 
         def scale_weights(q):
             values = w_grp[q][:].rearrange("p (n t) -> p n t", t=4)
@@ -498,19 +630,20 @@ def tile_relationalgraphconvolution_pa_kernel(
         def arranged_in(k):
             return k - 1 if k <= CATCH_UP else k - 2 - (k == STEPS - 2)
 
-        beside = {W_FIRST - 2: ("rel", 0)} if REL0_G else {}
-        for q in range(PASSES):
-            beside[W_FIRST + 2 * q] = ("w", q)
-        for it in range(1, IT - 1):
-            beside[W_FIRST + 2 * (PASSES + it - 1) + (it == IT - 3)] = ("rel", it)
-        rel_round = {job[1]: arranged_in(k) for k, job in beside.items() if job[0] == "rel"}
-        if not REL0_G:
-            rel_round[0] = REL0_AT
-        w_turn_at = {arranged_in(k) - W_AHEAD: job[1] for k, job in beside.items() if job[0] == "w"}
-        sums_turn_at = {t - 1: it for it, t in rel_round.items()}
+        windows = list(WINDOWS)
+        beside = {k: (job[0], int(job[1])) for k, job in zip(windows, JOBS.split())}
+        w_round = {W_TURN.get(job[1], arranged_in(k) - 1) + 1: job[1] for k, job in beside.items() if job[0] == "w"}
+        sums_turn_at = {arranged_in(k) - 1: job[1] for k, job in beside.items() if job[0] == "r"}
+        own = dict(OWN)
+        for t in own:
+            sums_turn_at[t - 1] = own[t]
         project_at = {t: it for it, t in enumerate(PROJECT_AT)}
-        node_at = {max((t - 1) * DEFER, GROUPS * it + 8): it for it, t in enumerate(PROJECT_AT + (29,))}
         left = list(range(len(PROJECT_AT), IT - 1))
+        complete = {}
+        for (it, r), (s, a) in place.items():
+            k = couple_of(it, r // RG)[0]
+            complete[k] = max(complete.get(k, 0), s)
+        couple_at = {(PAIR_AT[k] if paired(s) else s + UNIT_LAG): k for k, s in complete.items()}
 
         narrow_at = {t: [] for t in range(STEPS)}
         for s in range(STEPS - 1):
@@ -520,155 +653,213 @@ def tile_relationalgraphconvolution_pa_kernel(
                 narrow_at[s + 1 + (split and 2 * a >= len(tiles))].append((s, a))
         keep_at = {}
         for it in range(IT):
-            last = max(t for t in narrow_at for s, a in narrow_at[t] if s // GROUPS == it)
-            keep_at[max(last, GROUPS * it + 3) + 1] = it
+            last = max(t for t in narrow_at for s, a in narrow_at[t] if tile_of(s, a)[0] == it)
+            keep_at.setdefault(max(last, max(place[it, r][0] for r in range(R)) - KEEP_LEAD) + 1, []).append(it)
 
         def narrow_of_round(t):
             return [(s, a, v, j) for v in range(2) for s, a in narrow_at[t] for j in range(4)]
+
+        quantised = []
+
+        def quantise_due(t, below=99):
+            for t0, k in sorted(couple_at.items()):
+                if t0 <= t - QLAG and k not in quantised and k < below:
+                    quantise_couple(k)
+                    quantised.append(k)
 
         def finish(job):
             if job[0] == "w":
                 quantise_weights(job[1])
             else:
-                quantise_supports(job[1], 4)
+                quantise_relation_part(job[1])
+
+        def order_of(k):
+            return range(RG)
 
         def cross_step(k):
             n = RG - on_vector(k)
-            if n == RG and k <= HALVED:
+            if paired(k) and (k <= HALVED or n < RG):
+                for a in range(n):
+                    cross(k, a, 1)
+            elif n == RG and (paired(k) or k <= HALVED):
                 cross(k, 0, 2)
-                cross(k, 2, 2)
+                cross(k, 1 if paired(k) else 2, 2)
             elif n:
                 cross(k, 0, n)
 
         def arrange(k):
             n = RG - on_vector(k)
-            if k < 2:
-                for a in range(RG):
-                    if a < n:
-                        cross(k, a, 1)
-                    else:
-                        sort_and_sum(k, a)
-                    chores[RG * k + a]()
-                return
             job = beside.get(k)
-            if k == CATCH_UP + 1:
+            if k == CATCH_UP + 1 and arranged_in(k) not in VH:
                 cross_step(k - 1)
             cross_step(k)
+            if job and arranged_in(k) not in VH and k in covers:
+                quantise_due(arranged_in(k))
             if job and job[0] == "w":
-                pick_values(w_scale, scale_masked, job[1], 1)
-            elif job:
+                if job[1] in W_EXIT_V:
+                    empty_weights(job[1], nc.vector.tensor_copy)
+                cols = slice(4 * job[1], 4 * job[1] + 4)
+                nc.vector.tensor_copy(out=w_scale[:, cols], in_=factors[:, cols])
+            elif job and job[0] == "r":
                 collect_sums(job[1])
-            earlier = [j for j in beside if j < k]
-            if job and earlier:
-                finish(beside[max(earlier)])
+            if job and arranged_in(k) in finish_at:
+                finish(finish_at[arranged_in(k)])
+            if job and arranged_in(k) not in VH and k not in covers:
+                quantise_due(arranged_in(k))
+            if job and arranged_in(k) - 2 in own:
+                quantise_relation_part(own[arranged_in(k) - 2])
             for j in covers.get(k, ()):
                 cross_step(j)
-            if k == W_FIRST:
-                relation_part(0, nc.vector)
-            if k == W_FIRST + 2:
-                quantise_supports(0, 4)
             if job and job[0] == "w":
                 scale_weights(job[1])
             elif job:
                 relation_part(job[1], nc.gpsimd)
-            for a in range(n, RG):
-                sort_and_sum(k, a)
+            for a in order_of(k):
+                if a >= n:
+                    sort_and_sum(k, a)
 
         covers = {k: (k + 1,) for k in beside if COVER_FROM <= k + 1 < STEPS - 2}
         covers[STEPS - 2] = (STEPS - 3,)
         covered = [CATCH_UP] + [j for k in covers for j in covers[k]]
+        job_rounds = [arranged_in(k) for k in beside]
+        finish_at = {arranged_in(k) + 2: job for k, job in beside.items()}
 
         def clear(it):
             return lambda: nc.vector.memset(rep[it][:], 0.0)
 
-        def make_pick():
-            nc.vector.tensor_reduce(
-                out=pick[:], in_=ident[:].rearrange("p (g x) -> p x g", x=GROUP), axis=AXIS_X, op=ADD
-            )
+        def do(op, t):
+            kind, arg = op[0], op[1:]
+            s, a = (int(v) for v in arg.split(".")) if "." in arg else (None, None)
+            if op == "il":
+                interleave_features()
+            elif op == "cf":
+                nc.vector.memset(factor_cols[:], 0.0)
+            elif op == "cb":
+                collect_band()
+            elif op == "sf":
+                sort_factors()
+            elif op[:2] == "q@":
+                quantise_features(int(op[2]))
+            elif kind == "f":
+                cross_features(int(arg))
+            elif kind == "x":
+                cross(s, a, 1)
+            elif kind == "s":
+                sort_and_sum(s, a)
+            elif kind in "tT":
+                bank = turn(s, a)
+                empty(s, a, bank, nc.scalar.copy if kind == "t" else nc.vector.tensor_copy)
+                give_bank(bank)
+            elif kind == "n":
+                for v in range(2):
+                    for j in range(4):
+                        narrow_sum(s, a, v, j)
+            elif kind == "b":
+                band_sum(s, a)
+            elif kind == "c":
+                clear(int(arg))()
+            elif kind == "h":
+                quantise(s, 2 * a, 2)
+            elif kind == "q":
+                quantise(int(arg))
+            elif kind == "a":
+                aggregate(int(arg))
+            elif kind == "k":
+                keep_supports(int(arg))
+            elif kind == "w":
+                widen_weights(int(arg) % 2, int(arg) // 2)
+            elif kind == "F":
+                empty_scaled(int(arg))
+            elif kind == "Q":
+                quantise_weights(int(arg))
+            elif kind == "X":
+                cross_step(int(arg))
+            elif kind == "A":
+                arrange(int(arg))
+            elif kind == "u":
+                quantise_couple(int(arg))
+                quantised.append(int(arg))
 
-        chores = [interleave_features, make_pick, lambda: quantise_features(0), clear(0)]
-        chores.extend([clear(1), lambda: quantise_features(1), clear(2), lambda: None])
+        def load_step(s):
+            load(s, 4 if s < SINGLY else 2 if s <= HALVED else 1)
+            if s == ROWS_BEHIND:
+                load_factors()
+            for h in range(2):
+                if W_BEHIND[h] == s:
+                    nc.sync.dma_start(out=w_bytes[h][:], in_=Wb_bytes[h * P : (h + 1) * P, :])
 
         load_features()
-        load(0, 4)
-        load(1, 4)
-        for s in range(2, PREFETCH):
-            load(s, 2)
-
-        cross_features(0)
-        cross_features(1)
-        arrange(0)
-        for s in range(STEPS - 2):
-            it, phase = s // GROUPS - 1, s % GROUPS
-            if s == 0:
-                load_rows(rel_rows, relation_features[0])
-            if s in W_LOAD:
-                h = W_LOAD.index(s)
-                nc.sync.dma_start(out=w_bytes[h][:], in_=Wb_bytes[h * P : (h + 1) * P, :])
-            if s == W_LOAD[1]:
-                load_rows(scale_rows, Wb_scale.rearrange("o (r f) -> (o r) f", f=F))
+        for s in range(PREFETCH + HEAD_ROUNDS):
+            load_step(s)
+        for op in HEAD.split():
+            do(op, 0)
+        for s in range(HEAD_ROUNDS, STEPS - 2):
             if s + PREFETCH < STEPS:
-                load(s + PREFETCH, 2 if s + PREFETCH <= HALVED else 1)
+                load_step(s + PREFETCH)
 
             banks, later = [], []
+            if W_EARLY and s in w_round:
+                turn_weights(w_round[s])
+                if w_round[s] not in W_EXIT_V:
+                    empty_weights(w_round[s], nc.scalar.copy)
+            if s in FUSED_AT:
+                turn_weights(FUSED_AT[s])
             if s > BAND_UNTIL:
-                banks = [turn(s, a) for a in range(RG)]
-            by_vector = int(s in [arranged_in(k) + 1 for k in SWAPPED])
+                banks = {a: turn(s, a) for a in order_of(s)}
+                if SUMS_LATE and s - 1 in sums_turn_at:
+                    turn_sums(sums_turn_at[s - 1])
+            by_vector = int(s in SWAPPED)
             if by_vector:
                 empty(s, 0, banks[0], nc.vector.tensor_copy)
 
-            ahead = [k for k in range(1, STEPS) if arranged_in(k) == s and k not in covered]
-            early = s <= EARLY
-            if early:
-                arrange(ahead[0])
-            if s == 1:
-                for tile in rep[3:]:
-                    nc.vector.memset(tile[:], 0.0)
-            if s >= 1:
+            if s in VH:
+                for op in VH[s].split():
+                    do(op, s)
+            else:
                 quantise(s - 1)
-            if s == 3:
-                mask_rows(rel_masked, rel_rows, DR)
-            if s == 4:
-                pick_values(relf, rel_masked, 0, 2)
-            if s == REL0_AT and not REL0_G:
-                collect_sums(0)
-                mask_rows(scale_masked, scale_rows, F)
-            if s in node_at:
-                quantise_supports(node_at[s], 0, 4)
-            for k in ahead[early:]:
-                arrange(k)
-            for w in range(4):
-                if WIDEN_AT[w] == s and w not in WIDEN_S:
-                    widen_weights(w // 2, w % 2, False)
+                if s in own:
+                    collect_sums(own[s])
+                if s not in job_rounds:
+                    if s in finish_at:
+                        finish(finish_at[s])
+                    quantise_due(s)
+                for k in range(1, STEPS):
+                    if arranged_in(k) == s and k not in covered:
+                        arrange(k)
+                for op in VX.get(s, "").split():
+                    do(op, s)
+                if s - 1 in own:
+                    relation_part(own[s - 1], nc.vector)
 
             if s > BAND_UNTIL:
-                if it >= 0 and phase >= 2:
-                    later.append(turn_supports(it, 2 * (phase - 2)))
-                if s in w_turn_at:
-                    later.append(turn_weights(w_turn_at[s]))
-            if s in keep_at:
-                keep_sums(keep_at[s])
-                spread_sums(keep_at[s])
+                if s in couple_at:
+                    later.append(turn_supports(couple_at[s]))
+                if s == FACTORS_AT:
+                    later.append(turn_factors())
+                if not W_EARLY and s + 1 in w_round:
+                    turn_weights(w_round[s + 1])
+                    if w_round[s + 1] not in W_EXIT_V:
+                        later.append(lambda q=w_round[s + 1]: empty_weights(q, nc.scalar.copy))
+            for it in keep_at.get(s, ()):
+                keep_sums(it)
+                spread_sums(it)
             narrow = narrow_of_round(s)
             if s <= BAND_UNTIL:
-                for a in range(RG):
+                for j, a in enumerate(order_of(s)):
                     bank = turn(s, a)
                     empty(s, a, bank)
                     give_bank(bank)
-                    k = RG * s + a
+                    k = RG * s + j
                     if k in BAND_AT:
-                        band_sum(0, BAND_AT.index(k))
+                        band_sum(*band_tiles()[BAND_AT.index(k)])
             else:
-                for a in range(by_vector, RG):
+                for j, a in list(enumerate(order_of(s)))[by_vector:]:
                     empty(s, a, banks[a])
                     give_bank(banks[a])
-                    if a == by_vector + 1 and by_vector:
+                    if j == by_vector + 1 and by_vector:
                         give_bank(banks[0])
                 for copy_out in later:
                     copy_out()
-            for w in WIDEN_S:
-                if WIDEN_AT[w] == s:
-                    widen_weights(w // 2, w % 2, True)
             if s >= 2:
                 issue(narrow, EDGE if s not in keep_at else 0)
                 aggregate_half(s - 2, 0)
@@ -679,14 +870,14 @@ def tile_relationalgraphconvolution_pa_kernel(
                 project(project_at[s], all_passes, 4, 3)
                 store(project_at[s])
             issue(narrow, len(narrow))
-            if s in sums_turn_at:
+            if s in sums_turn_at and not SUMS_LATE:
                 turn_sums(sums_turn_at[s])
 
         s, it = STEPS - 2, IT - 1
+        first, second = 2 * it, 2 * it + 1
         banks = [turn(s, a) for a in range(RG)]
-        later = [turn_supports(it - 1, 0)]
+        later = [turn_supports(first - 1) if first - 1 not in sgn else lambda: None]
         quantise(s - 1)
-        quantise_supports(it - 1, 4)
         for a in range(RG):
             empty(s, a, banks[a])
             give_bank(banks[a])
@@ -694,42 +885,53 @@ def tile_relationalgraphconvolution_pa_kernel(
         issue(narrow, len(narrow) // 2)
         aggregate(s - 2)
         issue(narrow, len(narrow))
-        later.append(turn_supports(it - 1, 2))
         later[0]()
         keep_supports(s - 2)
         keep_sums(it)
         spread_sums(it)
         s = STEPS - 1
-        banks = [turn(s, a) for a in range(2)]
-        later[1]()
-        banks.extend(turn(s, a) for a in range(2, RG))
-        turn_sums(it)
-        quantise(s - 1)
-        aggregate(s - 2)
-        for a in range(RG):
-            empty(s, a, banks[a], nc.vector.tensor_copy if a in DRAIN_V else nc.scalar.copy)
-            give_bank(banks[a])
-        collect_sums(it)
-        aggregate(s - 1)
-        keep_supports(s - 2)
-        for k in left[:-1]:
-            project(k, all_passes, 4, 3)
-        quantise(s, 0, 2)
-        quantise(s, 2, 2)
-        keep_supports(s - 1)
-        for k in left[:-1]:
-            store(k)
-        quantise_supports(it - 1, 0, 4)
-        relation_part(it, nc.vector)
-        quantise_supports(it, 4)
-        for a0 in (0, 2):
-            aggregate(s, a0, 2)
-            keep_supports(s, a0, 2)
-        project(it - 1, all_passes, 4, 3)
-        for q in range(4):
-            turn_supports(it, q, 1, nc.vector.tensor_copy if q in LAST_V else nc.scalar.copy)()
-        store(it - 1)
-        for q in range(4):
-            quantise_supports(it, q, 1)
-        project(it, all_passes, 4, 3)
-        store(it)
+        held_banks = {}
+        for op in DRAIN.split():
+            kind, arg = op[0], op[1:]
+            copy = nc.vector.tensor_copy if kind in "EYZ" else nc.scalar.copy
+            if kind == "t":
+                held_banks[arg] = turn(s, int(arg))
+            elif kind in "eE":
+                empty(s, int(arg), held_banks[arg], copy)
+                give_bank(held_banks[arg])
+            elif op == "ts":
+                pass
+            elif kind == "S":
+                turn_sums(int(arg))
+            elif kind == "C":
+                collect_sums(int(arg))
+            elif kind == "R":
+                relation_part(int(arg), nc.vector)
+            elif kind == "r":
+                quantise_relation_part(int(arg))
+            elif kind == "q":
+                quantise(int(arg))
+            elif kind == "h":
+                quantise(s, 2 * int(arg), 2)
+            elif kind == "a":
+                aggregate(int(arg))
+            elif kind == "A":
+                aggregate(s, 2 * int(arg), 2)
+            elif kind == "k":
+                keep_supports(int(arg))
+            elif kind == "K":
+                keep_supports(s, 2 * int(arg), 2)
+            elif kind in "xX":
+                k, w0, n = (int(v) for v in arg.split("."))
+                held_banks[k, w0] = turn_supports(k, w0, n, nc.scalar.copy if kind == "x" else nc.vector.tensor_copy)
+            elif kind == "y":
+                k, w0 = (int(v) for v in arg.split("."))
+                held_banks[k, w0]()
+            elif kind == "u":
+                quantise_couple(*(int(v) for v in arg.split(".")))
+            elif kind == "p":
+                tile, passes = arg.split(".")
+                order = [int(q) for w in DRAIN.split() if w[:2] == "p" + tile for q in w[3:]]
+                project(int(tile), [int(q) for q in passes], order[0], order[-1])
+            elif kind in "zZ":
+                store(int(arg), copy)

@@ -24,10 +24,10 @@ LEAD = 128
 PASSES = F // 32
 PREFETCH = 5
 RAWS = 8
-PAIRED = 1
-HALVED = 9
+PAIRED = 2
+HALVED = 7
 FIRST_WINDOW = 7
-W_BEHIND = (4, 4)
+W_BEHIND = (4,5)
 ROWS_BEHIND = 2
 WIDEN_AT = (4, 4, 5, 5, 5, 5, 6, 6, 7, 7)
 W_ORDER = (0, 1, 2, 3, 4, 5)
@@ -36,7 +36,7 @@ EARLY = 4
 BAND_UNTIL = 2
 BAND_AT = ()
 CATCH_UP = 8
-EXTRA_V = {3: 1}
+EXTRA_V = {0:1,1:1,3:1}
 PROJECT_AT = (20, 22, 24, 26, 28)
 COVER_FROM = 14
 SPLIT_FROM = 4
@@ -46,6 +46,9 @@ W_EXIT_V = ()
 W_EARLY = 0
 JOBS = "w3 w4 w5 r0 r1 r2 r3 r4 r5 r6"
 RC = 4
+PLAIN_AT = {}
+UNSPLIT = 0
+WG = 3
 NC = 10
 SUMS_LATE = 0
 WINDOWS = (13, 15, 17, 19, 21, 23, 25, 27, 30, 31)
@@ -53,13 +56,13 @@ FUSED_AT = {6: 0, 8: 1, 10: 2}
 PAIR_AT = (5, 7, 9, 11)
 W_TURN = {}
 FIRSTP = "40"
-DRAIN = "t0 t1 t2 t3 S7 q30 a29 e0 e1 e2 E3 a30 k29 h0 h1 p5.45 A0 k30 x14.0.2 A1 K0 K1 y14.0 C7 u12.0.2 r6 u13.0.2 p5.0123 R7 x15.0.2 y15.0 z5 p6.450123 u14.0.2 r7 u15.0.2 z6 p7.024513 z7"
+DRAIN = "t0 t1 t2 t3 S7 q30 a29 e0 e1 e2 E3 a30 k29 h0 h1 p5.45 A0 k30 x14.0.2 A1 K0 K1 y14.0 C7 u12.0.2 r6 u13.0.2 p5.0123 R7 x15.0.2 y15.0 z5 p6.450123 u14.0.2 r7 u15.0.2 z6 P024513 L"
 PAIR_LAG = 4
 VX = {}
 OWN = ()
-HEAD = "f0 f1 x0.0 il x0.1 t0.0 t0.1 q@0 x0.2 t0.2 c0 x0.3 t0.3 c1 q@1 c2 x1.0 x1.1 b0.0 t1.0 t1.1 h0.0 n0.1 b0.2 x1.2 x1.3 c3 t1.2 t1.3 h0.1 x2.0 x2.1 n0.3 b1.0 t2.0 t2.1 a0 cf h1.0 x2.2 x2.3 n1.1 t2.2 t2.3 k0 b1.2 h1.1 sf x3.0 x3.1 h2.0 n1.3 t3.0 t3.1 a1 x3.2 s3.3 cb n2.0 n2.1 t3.2 t3.3 k1 n2.2 n2.3 h2.1 x4.0 x4.1 c4 c5 x4.2 x4.3 c6 c7"
+HEAD = "f0 f1 x0.0 il x0.1 t0.0 t0.1 q@0 x0.2 t0.2 c0 s0.3 t0.3 c1 q@1 c2 x1.0 x1.1 b0.0 t1.0 t1.1 h0.0 n0.1 b0.2 x1.2 s1.3 c3 t1.2 t1.3 h0.1 x2.0 x2.1 b1.0 t2.0 t2.1 a0 cf h1.0 x2.2 x2.3 n1.1 t2.2 t2.3 k0 b1.2 h1.1 sf x3.0 x3.1 h2.0 t3.0 t3.1 a1 x3.2 s3.3 cb n2.0 n2.1 t3.2 t3.3 k1 n2.2 n2.3 h2.1 x4.0 x4.1 c4 c5 x4.2 x4.3 c6 c7"
 HEAD_ROUNDS = 4
-VH = {4: "w0 q3 w1 x5.0 x5.1 w2 x5.2 x5.3", 5: "q4 w3 w4 X6 w5", 6: "F0 q5 X7 w6 Q0", 7: "X8 q6 u0 w7 X9", 8: "F1 q7 X10 w8 Q1", 9: "q8 X11 u1 w9", 10: "F2 q9 X12 Q2"}
+VH = {4: "w0 q3 x5.0 x5.1 w2 x5.2 x5.3 w4", 5: "q4 w1 w3 X6 w5", 6: "F0 q5 X7 w6 Q0", 7: "X8 q6 u0 w7 X9", 8: "F1 q7 X10 w8 Q1", 9: "q8 X11 u1 w9", 10: "F2 q9 X12 Q2"}
 FACTORS_AT = 4
 SINGLY = 1
 Q_FIRST = 1
@@ -90,7 +93,7 @@ def paired(s):
 
 def tile_of(s, a):
     if paired(s):
-        return a % 2, (2 * s + a // 2 - RG) % R
+        return s // (2 * GROUPS) * 2 + a % 2, (2 * s + a // 2 - RG) % R
     return s // GROUPS, GROUP_AT[s % GROUPS] * RG + a
 
 
@@ -129,6 +132,7 @@ def tile_relationalgraphconvolution_pa_kernel(
         four = ctx.enter_context(tc.tile_pool(name="four", bufs=4))
         rcp = ctx.enter_context(tc.tile_pool(name="rcp", bufs=RC))
         ncp = ctx.enter_context(tc.tile_pool(name="ncp", bufs=NC))
+        wgp = ctx.enter_context(tc.tile_pool(name="wgp", bufs=WG))
         sgnp = ctx.enter_context(tc.tile_pool(name="sgnp", bufs=SGN))
         psum = ctx.enter_context(tc.psum_pool(name="psum", bufs=1))
         ctx.enter_context(tc.manual_schedule())
@@ -190,7 +194,7 @@ def tile_relationalgraphconvolution_pa_kernel(
 
         def couple_of(it, g):
             if paired(GROUPS * it):
-                return (g + 1) % GROUPS, it
+                return it // 2 * GROUPS + (g + 1) % GROUPS, it % 2
             return 2 * it + GROUP_AT.index(g) // 2, GROUP_AT.index(g) % 2
 
         free_banks = list(range(BANKS - 2))
@@ -545,10 +549,10 @@ def tile_relationalgraphconvolution_pa_kernel(
             r_scales[it] = rcp.tile([P, 2 * P], U8, name="r_scales", align_bytes=64)
             nc.vector.quantize_mx(out=r_codes[it][:].bitcast(FP8X4), scales=r_scales[it][:], in_=sgr[it][:])
 
-        def project(it, passes, first, last):
+        def project(it, passes, first, last, n0=0, n1=NB):
             for q in passes:
                 if q == first:
-                    obank[it] = take_bank()
+                    obank[it, n0] = take_bank()
                 if q < GROUPS:
                     k, w = couple_of(it, q)
                     cols = slice(w * P, (w + 1) * P)
@@ -557,24 +561,24 @@ def tile_relationalgraphconvolution_pa_kernel(
                     cols = slice((q - GROUPS) * P, (q - GROUPS + 1) * P)
                     words, exps = r_codes[it][:, cols], r_scales[it][:, cols]
                 nc.tensor.matmul_mx(
-                    out=obank[it][:, 0:NB],
+                    out=obank[it, n0][:, n0:n1],
                     lhsT=words.bitcast(FP8X4),
                     lhsT_scale=exps,
-                    rhs=w_codes[:, q * NB : (q + 1) * NB].bitcast(FP8X4),
-                    rhs_scale=w_scales[:, q * NB : (q + 1) * NB],
+                    rhs=w_codes[:, q * NB + n0 : q * NB + n1].bitcast(FP8X4),
+                    rhs_scale=w_scales[:, q * NB + n0 : q * NB + n1],
                     start=(q == first),
                     stop=(q == last),
                 )
 
-        def store(it, copy=nc.scalar.copy):
-            res = three.tile([P, NB], F32, name="res", align_bytes=64)
-            copy(out=res[:], in_=obank[it][:, 0:NB])
-            give_bank(obank[it])
+        def store(it, copy=nc.scalar.copy, n0=0, n1=NB, queue=nc.sync):
+            res = four.tile([P, n1 - n0], F32, name="res", align_bytes=64)
+            copy(out=res[:], in_=obank[it, n0][:, n0:n1])
+            give_bank(obank[it, n0])
             if paired(GROUPS * it):
                 rows = out[0, it // 2 * 2 * P : (it // 2 + 1) * 2 * P, :].rearrange("(i h) n -> h i n", h=2)[it % 2]
             else:
                 rows = out[0, it * P : (it + 1) * P, :]
-            nc.sync.dma_start(out=rows, in_=res[:])
+            queue.dma_start(out=rows[:, n0:n1], in_=res[:])
 
         def widen_weights(h, g):
             rows = w_bytes[h][:].rearrange("p (r k) -> p r k", k=F)
@@ -595,7 +599,7 @@ def tile_relationalgraphconvolution_pa_kernel(
                     nc.tensor.transpose(w_bank[q][:, k0 : k0 + P], w_val[h][:].bitcast(F32)[:, w0 : w0 + P], ident[:])
 
         def empty_weights(q, copy):
-            w_grp[q] = three.tile([P, 4 * NB], BF16, name="w_grp", align_bytes=64)
+            w_grp[q] = wgp.tile([P, 4 * NB], BF16, name="w_grp", align_bytes=64)
             copy(
                 out=w_grp[q][:].bitcast(F32).rearrange("p (n u) -> p n u", u=2),
                 in_=w_bank[q][:].rearrange("p (u n) -> p n u", u=2),
@@ -603,7 +607,7 @@ def tile_relationalgraphconvolution_pa_kernel(
             give_bank(w_bank[q])
 
         def empty_scaled(q):
-            w_grp[q] = three.tile([P, 4 * NB], BF16, name="w_grp", align_bytes=64)
+            w_grp[q] = wgp.tile([P, 4 * NB], BF16, name="w_grp", align_bytes=64)
             nc.vector.tensor_tensor(
                 out=w_grp[q][:].rearrange("p (n u e) -> p n u e", u=2, e=2),
                 in0=w_bank[q][:].bitcast(BF16).rearrange("p (u n e) -> p n u e", u=2, e=2),
@@ -611,6 +615,15 @@ def tile_relationalgraphconvolution_pa_kernel(
                 op=MULT,
             )
             give_bank(w_bank[q])
+
+        def scale_here(q):
+            values = w_grp[q][:].rearrange("p (n t) -> p n t", t=4)
+            nc.vector.tensor_tensor(
+                out=values,
+                in0=values,
+                in1=factors[:, q * 4 : (q + 1) * 4].unsqueeze(1).to_broadcast([P, NB, 4]),
+                op=MULT,
+            )
 
         def scale_weights(q):
             values = w_grp[q][:].rearrange("p (n t) -> p n t", t=4)
@@ -643,7 +656,7 @@ def tile_relationalgraphconvolution_pa_kernel(
         for (it, r), (s, a) in place.items():
             k = couple_of(it, r // RG)[0]
             complete[k] = max(complete.get(k, 0), s)
-        couple_at = {(PAIR_AT[k] if paired(s) else s + UNIT_LAG): k for k, s in complete.items()}
+        couple_at = {(PAIR_AT[k] if k < len(PAIR_AT) else s + UNIT_LAG): k for k, s in complete.items()}
 
         narrow_at = {t: [] for t in range(STEPS)}
         for s in range(STEPS - 1):
@@ -768,6 +781,17 @@ def tile_relationalgraphconvolution_pa_kernel(
                 keep_supports(int(arg))
             elif kind == "w":
                 widen_weights(int(arg) % 2, int(arg) // 2)
+            elif kind == "W":
+                turn_weights(int(arg))
+                empty_weights(int(arg), nc.scalar.copy)
+            elif kind == "G":
+                turn_factors()()
+            elif kind == "U":
+                turn_supports(int(arg))()
+            elif kind == "g":
+                aggregate_half(s, a)
+            elif kind == "H":
+                scale_here(int(arg))
             elif kind == "F":
                 empty_scaled(int(arg))
             elif kind == "Q":
@@ -836,6 +860,9 @@ def tile_relationalgraphconvolution_pa_kernel(
                     later.append(turn_supports(couple_at[s]))
                 if s == FACTORS_AT:
                     later.append(turn_factors())
+                if s in PLAIN_AT:
+                    turn_weights(PLAIN_AT[s])
+                    later.append(lambda q=PLAIN_AT[s]: empty_weights(q, nc.scalar.copy))
                 if not W_EARLY and s + 1 in w_round:
                     turn_weights(w_round[s + 1])
                     if w_round[s + 1] not in W_EXIT_V:
@@ -863,7 +890,8 @@ def tile_relationalgraphconvolution_pa_kernel(
             if s >= 2:
                 issue(narrow, EDGE if s not in keep_at else 0)
                 aggregate_half(s - 2, 0)
-                issue(narrow, len(narrow) - EDGE)
+                if len(narrow) > UNSPLIT:
+                    issue(narrow, len(narrow) - EDGE)
                 aggregate_half(s - 2, 1)
                 keep_supports(s - 2)
             if s in project_at:
@@ -933,5 +961,13 @@ def tile_relationalgraphconvolution_pa_kernel(
                 tile, passes = arg.split(".")
                 order = [int(q) for w in DRAIN.split() if w[:2] == "p" + tile for q in w[3:]]
                 project(int(tile), [int(q) for q in passes], order[0], order[-1])
+            elif kind == "P":
+                order = [int(q) for w in DRAIN.split() if w[0] == "P" for q in w[1:]]
+                for q in arg:
+                    for n0 in (0, P):
+                        project(it, [int(q)], order[0], order[-1], n0, n0 + P)
+            elif op == "L":
+                store(it, nc.vector.tensor_copy, 0, P)
+                store(it, nc.scalar.copy, P, NB, nc.scalar)
             elif kind in "zZ":
                 store(int(arg), copy)

@@ -18,7 +18,7 @@ GROUP_AT = (0, 2, 1, 3)
 GROUP = 8
 RUN = 16
 BANKS = 8
-EDGE = 4
+EDGE = 8
 NARROW, BAND, VECTOR = range(3)
 LEAD = 128
 PASSES = F // 32
@@ -47,7 +47,7 @@ W_EARLY = 0
 JOBS = "w3 w4 w5 r0 r1 r2 r3 r4 r5 r6"
 RC = 4
 PLAIN_AT = {}
-UNSPLIT = 0
+UNSPLIT = 16
 WG = 3
 NC = 10
 SUMS_LATE = 0

@@ -1,4 +1,5 @@
 from contextlib import ExitStack
+from functools import partial
 
 import concourse.mybir as mybir
 from concourse.masks import make_identity
@@ -14,65 +15,31 @@ IT = N // P
 RG = 4
 GROUPS = R // RG
 STEPS = IT * GROUPS
-GROUP_AT = (0, 2, 1, 3)
+PASSES = F // 32
 GROUP = 8
 RUN = 16
 BANKS = 8
-EDGE = 8
-NARROW, BAND, VECTOR = range(3)
 LEAD = 128
-PASSES = F // 32
+NARROW, BAND, VECTOR = range(3)
+
+PAIRED = 4
+PAIRED_STEPS = PAIRED * GROUPS
+GROUP_AT = (0, 2, 1, 3)
 PREFETCH = 5
-RAWS = 8
-PAIRED = 2
+HEAD = 4
 HALVED = 7
-FIRST_WINDOW = 7
-W_BEHIND = (4,5)
-ROWS_BEHIND = 2
-WIDEN_AT = (4, 4, 5, 5, 5, 5, 6, 6, 7, 7)
-W_ORDER = (0, 1, 2, 3, 4, 5)
-CONST_AT = 4
-EARLY = 4
-BAND_UNTIL = 2
-BAND_AT = ()
-CATCH_UP = 8
-EXTRA_V = {0:1,1:1,3:1}
-PROJECT_AT = (20, 22, 24, 26, 28)
-COVER_FROM = 14
-SPLIT_FROM = 4
-SHORT = (13, 15, 17)
-SWAPPED = (12, 14, 16)
-W_EXIT_V = ()
-W_EARLY = 0
-JOBS = "w3 w4 w5 r0 r1 r2 r3 r4 r5 r6"
-RC = 4
-PLAIN_AT = {}
-UNSPLIT = 16
-WG = 3
-NC = 10
-SUMS_LATE = 0
-WINDOWS = (13, 15, 17, 19, 21, 23, 25, 27, 30, 31)
-FUSED_AT = {6: 0, 8: 1, 10: 2}
-PAIR_AT = (5, 7, 9, 11)
-W_TURN = {}
-FIRSTP = "40"
-DRAIN = "t0 t1 t2 t3 S7 q30 a29 e0 e1 e2 E3 a30 k29 h0 h1 p5.45 A0 k30 x14.0.2 A1 K0 K1 y14.0 C7 u12.0.2 r6 u13.0.2 p5.0123 R7 x15.0.2 y15.0 z5 p6.450123 u14.0.2 r7 u15.0.2 z6 P024513 L"
-PAIR_LAG = 4
-VX = {}
-OWN = ()
-HEAD = "f0 f1 x0.0 il x0.1 t0.0 t0.1 q@0 x0.2 t0.2 c0 s0.3 t0.3 c1 q@1 c2 x1.0 x1.1 b0.0 t1.0 t1.1 h0.0 n0.1 b0.2 x1.2 s1.3 c3 t1.2 t1.3 h0.1 x2.0 x2.1 b1.0 t2.0 t2.1 a0 cf h1.0 x2.2 x2.3 n1.1 t2.2 t2.3 k0 b1.2 h1.1 sf x3.0 x3.1 h2.0 t3.0 t3.1 a1 x3.2 s3.3 cb n2.0 n2.1 t3.2 t3.3 k1 n2.2 n2.3 h2.1 x4.0 x4.1 c4 c5 x4.2 x4.3 c6 c7"
-HEAD_ROUNDS = 4
-VH = {4: "w0 q3 x5.0 x5.1 w2 x5.2 x5.3 w4", 5: "q4 w1 w3 X6 w5", 6: "F0 q5 X7 w6 Q0", 7: "X8 q6 u0 w7 X9", 8: "F1 q7 X10 w8 Q1", 9: "q8 X11 u1 w9", 10: "F2 q9 X12 Q2"}
-FACTORS_AT = 4
-SINGLY = 1
-Q_FIRST = 1
-KEEP_LEAD = 0
-DRAIN_V = (0,)
-LAST_V = 0
-UNIT_LAG = 4
-QLAG = 1
-SGN = 3
-CLEAR_AT = 1
+FACTORS_BEHIND = 2
+W_BEHIND = (4, 5)
+HEAD_SUMS = (0, 1, 3)
+FIRST_WINDOW = 13
+WINDOWS = tuple(range(FIRST_WINDOW, STEPS - 4, 2)) + (STEPS - 2, STEPS - 1)
+ON_GPSIMD = 3
+FIRST_SCALED = 6
+FIRST_COUPLE = 5
+FIRST_PROJECT = FIRST_WINDOW + 2 * ON_GPSIMD + 1
+EDGE = 8
+SPLIT_UNTIL = STEPS - 6
+BAND_FROM = 96
 
 F32 = mybir.dt.float32
 BF16 = mybir.dt.bfloat16
@@ -88,7 +55,7 @@ FLOPS = 2 * (R * N * N * DE + N * R * F * NB)
 
 
 def paired(s):
-    return s < 2 * GROUPS * PAIRED
+    return s < PAIRED_STEPS
 
 
 def tile_of(s, a):
@@ -103,20 +70,29 @@ def row_start(s, a):
     return LEAD + a * (LEAD + N)
 
 
+def couple_of(it, g):
+    if it < PAIRED:
+        return it // 2 * GROUPS + (g + 1) % GROUPS, it % 2
+    return 2 * it + GROUP_AT.index(g) // 2, GROUP_AT.index(g) % 2
+
+
 def on_vector(s):
     if s in WINDOWS:
-        return RG - (s in SHORT)
-    return EXTRA_V.get(s, 0)
+        return RG - (s in WINDOWS[:ON_GPSIMD])
+    return int(s in HEAD_SUMS)
 
 
-def band_tiles():
-    return [(s, a) for s in range(2) for a in range(RG) if tile_of(s, a)[0] == 0]
+BAND_TILES = ((0, 0), (0, 2), (1, 0), (1, 2))
 
 
 def summed_by(s, a):
     if a >= RG - on_vector(s):
         return VECTOR
-    return BAND if (s, a) in band_tiles() else NARROW
+    return BAND if (s, a) in BAND_TILES else NARROW
+
+
+def arranged_in(k):
+    return k - 2 - (k == STEPS - 2)
 
 
 def tile_relationalgraphconvolution_pa_kernel(
@@ -125,15 +101,14 @@ def tile_relationalgraphconvolution_pa_kernel(
     nc = tc.nc
     with ExitStack() as ctx:
         keep = ctx.enter_context(tc.tile_pool(name="keep", bufs=1))
-        rawp = ctx.enter_context(tc.tile_pool(name="rawp", bufs=RAWS))
-        onep = ctx.enter_context(tc.tile_pool(name="onep", bufs=8))
-        two = ctx.enter_context(tc.tile_pool(name="two", bufs=2))
+        rawp = ctx.enter_context(tc.tile_pool(name="rawp", bufs=PREFETCH + 3))
+        onep = ctx.enter_context(tc.tile_pool(name="onep", bufs=2 * RG))
         three = ctx.enter_context(tc.tile_pool(name="three", bufs=3))
         four = ctx.enter_context(tc.tile_pool(name="four", bufs=4))
-        rcp = ctx.enter_context(tc.tile_pool(name="rcp", bufs=RC))
-        ncp = ctx.enter_context(tc.tile_pool(name="ncp", bufs=NC))
-        wgp = ctx.enter_context(tc.tile_pool(name="wgp", bufs=WG))
-        sgnp = ctx.enter_context(tc.tile_pool(name="sgnp", bufs=SGN))
+        rcp = ctx.enter_context(tc.tile_pool(name="rcp", bufs=4))
+        ncp = ctx.enter_context(tc.tile_pool(name="ncp", bufs=10))
+        wgp = ctx.enter_context(tc.tile_pool(name="wgp", bufs=3))
+        sgnp = ctx.enter_context(tc.tile_pool(name="sgnp", bufs=3))
         psum = ctx.enter_context(tc.psum_pool(name="psum", bufs=1))
         ctx.enter_context(tc.manual_schedule())
 
@@ -173,29 +148,10 @@ def tile_relationalgraphconvolution_pa_kernel(
         w_val = [keep.tile([P, R * F], BF16, name="w_val%d" % h, align_bytes=64) for h in range(2)]
         w_codes = keep.tile([P, PASSES * NB], U32, name="w_codes", align_bytes=64)
         w_scales = keep.tile([P, PASSES * NB], U8, name="w_scales", align_bytes=64)
-        n_codes = {}
-        n_scales = {}
 
-        raw = {}
-        window = {}
-        grp = {}
-        codes = {}
-        scales = {}
-        mx = {}
-        sums = {}
-        sup = {}
-        sgn = {}
-        sgr = {}
-        r_codes = {}
-        r_scales = {}
-        obank = {}
-        w_grp = {}
-        w_bank = {}
-
-        def couple_of(it, g):
-            if paired(GROUPS * it):
-                return it // 2 * GROUPS + (g + 1) % GROUPS, it % 2
-            return 2 * it + GROUP_AT.index(g) // 2, GROUP_AT.index(g) % 2
+        raw, window, grp, codes, scales, mx = {}, {}, {}, {}, {}, {}
+        turned, sums, sup, sgn, sgr, obank = {}, {}, {}, {}, {}, {}
+        n_codes, n_scales, r_codes, r_scales, w_grp, w_bank = {}, {}, {}, {}, {}, {}
 
         free_banks = list(range(BANKS - 2))
         held = {}
@@ -212,34 +168,36 @@ def tile_relationalgraphconvolution_pa_kernel(
         sums_bank = psum.tile([P, 512], F32, name="bank%d" % (BANKS - 1))
         first_sums = psum.tile([P, 512], F32, name="bank%d" % (BANKS - 2))
         held[BANKS - 2] = first_sums
-        turned = {}
 
         def rows_of(s, a0, n, shift):
             pitch = LEAD + (2 * N if paired(s) else N)
             first = row_start(s, a0) + shift
             return raw[s][:, first : first + n * pitch].rearrange("p (a q) -> p a q", q=pitch)
 
-        def load(s, pieces=1):
+        def load(s):
             raw[s] = rawp.tile([P, LEAD + RG * (LEAD + N)], BF16, name="raw", align_bytes=256)
             it, r0 = tile_of(s, 0)
-            if paired(s):
-                rows = adj[0, r0 : r0 + 2, it * P : (it + 2) * P, :].rearrange("r (i h) j -> i r (h j)", h=2)
-                if pieces == 4:
-                    for a in range(RG):
-                        nc.sync.dma_start(
-                            out=raw[s][:, row_start(s, a) : row_start(s, a) + N], in_=rows[:, a // 2, a % 2 * N : (a % 2 + 1) * N]
-                        )
-                    return
-                n = 2 // pieces
-                for a0 in range(0, 2, n):
-                    nc.sync.dma_start(out=rows_of(s, 2 * a0, n, 0)[:, :, 0 : 2 * N], in_=rows[:, a0 : a0 + n])
+            if not paired(s):
+                rows = adj[0, r0 : r0 + RG, it * P : (it + 1) * P, :].rearrange("r i j -> i r j")
+                nc.sync.dma_start(out=rows_of(s, 0, RG, 0)[:, :, 0:N], in_=rows)
                 return
-            n = RG // pieces
-            for a0 in range(0, RG, n):
-                nc.sync.dma_start(
-                    out=rows_of(s, a0, n, 0)[:, :, 0:N],
-                    in_=adj[0, r0 + a0 : r0 + a0 + n, it * P : (it + 1) * P, :].rearrange("r i j -> i r j"),
-                )
+            rows = adj[0, r0 : r0 + 2, it * P : (it + 2) * P, :].rearrange("r (i h) j -> i r (h j)", h=2)
+            if s == 0:
+                for a in range(RG):
+                    dst = raw[s][:, row_start(s, a) : row_start(s, a) + N]
+                    nc.sync.dma_start(out=dst, in_=rows[:, a // 2, a % 2 * N : (a % 2 + 1) * N])
+                return
+            n = 1 if s <= HALVED else 2
+            for r in range(0, 2, n):
+                nc.sync.dma_start(out=rows_of(s, 2 * r, n, 0)[:, :, 0 : 2 * N], in_=rows[:, r : r + n])
+
+        def load_step(s):
+            load(s)
+            if s == FACTORS_BEHIND:
+                load_factors()
+            if s in W_BEHIND:
+                h = W_BEHIND.index(s)
+                nc.sync.dma_start(out=w_bytes[h][:], in_=Wb_bytes[h * P : (h + 1) * P, :])
 
         def load_features():
             runs = node_features[0].rearrange("(c b u x e) d -> c u b x (e d)", c=2, u=2, x=8, e=2)
@@ -294,7 +252,9 @@ def tile_relationalgraphconvolution_pa_kernel(
             src = node_rows.rearrange("p (a m x e) -> p e a m x", a=RG, x=GROUP, e=2)
             for u in range(2):
                 nc.vector.tensor_copy(
-                    out=factor_cols[0:GROUPS, u * 2 * P : (u + 1) * 2 * P].rearrange("p (e a q x) -> p e a q x", e=2, a=RG, x=GROUP),
+                    out=factor_cols[0:GROUPS, u * 2 * P : (u + 1) * 2 * P].rearrange(
+                        "p (e a q x) -> p e a q x", e=2, a=RG, x=GROUP
+                    ),
                     in_=src[:, :, :, u:8:2, :],
                 )
             for p0, rows in ((32, rel_rows), (64, relf_rows)):
@@ -382,9 +342,6 @@ def tile_relationalgraphconvolution_pa_kernel(
                 in_=grp[s][:, a0 * N : (a0 + n) * N],
             )
 
-        def aggregate_half(s, half):
-            aggregate(s, 0, RG, range(2 * half, 2 * half + 2))
-
         def aggregate(s, a0=0, n=RG, tiles=None):
             if (s, a0) not in mx:
                 mx[s, a0] = take_bank()
@@ -421,18 +378,17 @@ def tile_relationalgraphconvolution_pa_kernel(
                 )
             give_bank(mx[s, a0])
 
-        def turn_supports(k, w0=0, n=2, copy=nc.scalar.copy):
-            if w0 == 0:
-                sgn[k] = sgnp.tile([P, 1024], BF16, name="sgn", align_bytes=64)
+        def turn_couple(k):
+            sgn[k] = sgnp.tile([P, 1024], BF16, name="sgn", align_bytes=64)
             bank = take_bank()
-            for j in range(2 * n):
-                c0 = (2 * w0 + j) * P
-                nc.tensor.transpose(bank[:, j * P : (j + 1) * P], sup[k][:].bitcast(F32)[:, c0 : c0 + P], ident[:])
+            for j in range(4):
+                cols = slice(j * P, (j + 1) * P)
+                nc.tensor.transpose(bank[:, cols], sup[k][:].bitcast(F32)[:, cols], ident[:])
 
             def copy_out():
-                copy(
-                    out=sgn[k][:, w0 * 512 : (w0 + n) * 512].bitcast(F32).rearrange("p (b i u) -> p b i u", b=n, u=2),
-                    in_=bank[:, 0 : n * 256].rearrange("p (b u i) -> p b i u", b=n, u=2),
+                nc.scalar.copy(
+                    out=sgn[k][:].bitcast(F32).rearrange("p (w i u) -> p w i u", w=2, u=2),
+                    in_=bank[:].rearrange("p (w u i) -> p w i u", w=2, u=2),
                 )
                 give_bank(bank)
 
@@ -451,16 +407,12 @@ def tile_relationalgraphconvolution_pa_kernel(
             )
 
         def issue(narrow, n):
-            n = max(n, 0)
             for item in narrow[:n]:
                 narrow_sum(*item)
             narrow[:n] = []
 
-        def turned_sums(it):
-            return turned[it][:, 0 : 2 * P]
-
         def band_sum(s, a):
-            it, r = tile_of(s, a)
+            r = tile_of(s, a)[1]
             for c in range(2):
                 words = grp[s][:, a * N + c * 512 : a * N + (c + 1) * 512].rearrange("p (i u e) -> p u i e", u=2, e=2)
                 for u in range(2):
@@ -468,8 +420,8 @@ def tile_relationalgraphconvolution_pa_kernel(
                         first_sums[:, 0 : 2 * P].rearrange("p (i e) -> p i e", e=2),
                         lhsT=band[:, P - GROUP * (r + 1) : 2 * P - GROUP * (r + 1)],
                         rhs=words[:, u],
-                        start=(s == 0 and a == 0 and c == 0 and u == 0),
-                        stop=((s, a) == band_tiles()[-1] and c == 1 and u == 1),
+                        start=((s, a) == BAND_TILES[0] and c == 0 and u == 0),
+                        stop=((s, a) == BAND_TILES[-1] and c == 1 and u == 1),
                     )
 
         def columns_of(it, kind):
@@ -496,7 +448,7 @@ def tile_relationalgraphconvolution_pa_kernel(
             turned[it] = take_bank()
             for v in range(last + 1):
                 nc.tensor.matmul(
-                    turned_sums(it)[:, v * P : (v + 1) * P] if v < 2 else turned_sums(it)[:, 0 : 2 * P : 2],
+                    turned[it][:, v * P : (v + 1) * P] if v < 2 else turned[it][:, 0 : 2 * P : 2],
                     lhsT=rep[it][:, v * P : (v + 1) * P],
                     rhs=ident[:],
                     start=(v == 0),
@@ -507,8 +459,8 @@ def tile_relationalgraphconvolution_pa_kernel(
         def collect_band():
             sums[0] = three.tile([P, P], F32, name="sums", align_bytes=64)
             nc.vector.tensor_reduce(
-                out=sums[0][96:P, :],
-                in_=first_sums[96:P, 0 : 2 * P].rearrange("p (i u) -> p i u", u=2),
+                out=sums[0][BAND_FROM:P, :],
+                in_=first_sums[BAND_FROM:P, 0 : 2 * P].rearrange("p (i u) -> p i u", u=2),
                 axis=AXIS_X,
                 op=ADD,
             )
@@ -517,10 +469,10 @@ def tile_relationalgraphconvolution_pa_kernel(
         def collect_sums(it):
             if it > 0:
                 sums[it] = three.tile([P, P], F32, name="sums", align_bytes=64)
-            p1 = P if it > 0 else 96
+            p1 = P if it > 0 else BAND_FROM
             nc.vector.tensor_reduce(
                 out=sums[it][0:p1, :],
-                in_=turned_sums(it)[0:p1].rearrange("p (i u) -> p i u", u=2),
+                in_=turned[it][0:p1, 0 : 2 * P].rearrange("p (i u) -> p i u", u=2),
                 axis=AXIS_X,
                 op=ADD,
             )
@@ -535,23 +487,19 @@ def tile_relationalgraphconvolution_pa_kernel(
                 op=MULT,
             )
 
-        def quantise_couple(k, w0=0, n=2):
-            if k not in n_codes:
-                n_codes[k] = ncp.tile([P, 2 * P], U32, name="n_codes", align_bytes=64)
-                n_scales[k] = ncp.tile([P, 2 * P], U8, name="n_scales", align_bytes=64)
-            cols = slice(w0 * P, (w0 + n) * P)
-            nc.vector.quantize_mx(
-                out=n_codes[k][:, cols].bitcast(FP8X4), scales=n_scales[k][:, cols], in_=sgn[k][:, w0 * 512 : (w0 + n) * 512]
-            )
+        def quantise_couple(k):
+            n_codes[k] = ncp.tile([P, 2 * P], U32, name="n_codes", align_bytes=64)
+            n_scales[k] = ncp.tile([P, 2 * P], U8, name="n_scales", align_bytes=64)
+            nc.vector.quantize_mx(out=n_codes[k][:].bitcast(FP8X4), scales=n_scales[k][:], in_=sgn[k][:])
 
         def quantise_relation_part(it):
             r_codes[it] = rcp.tile([P, 2 * P], U32, name="r_codes", align_bytes=64)
             r_scales[it] = rcp.tile([P, 2 * P], U8, name="r_scales", align_bytes=64)
             nc.vector.quantize_mx(out=r_codes[it][:].bitcast(FP8X4), scales=r_scales[it][:], in_=sgr[it][:])
 
-        def project(it, passes, first, last, n0=0, n1=NB):
+        def project(it, passes, order, n0=0, n1=NB):
             for q in passes:
-                if q == first:
+                if q == order[0]:
                     obank[it, n0] = take_bank()
                 if q < GROUPS:
                     k, w = couple_of(it, q)
@@ -566,21 +514,21 @@ def tile_relationalgraphconvolution_pa_kernel(
                     lhsT_scale=exps,
                     rhs=w_codes[:, q * NB + n0 : q * NB + n1].bitcast(FP8X4),
                     rhs_scale=w_scales[:, q * NB + n0 : q * NB + n1],
-                    start=(q == first),
-                    stop=(q == last),
+                    start=(q == order[0]),
+                    stop=(q == order[-1]),
                 )
 
         def store(it, copy=nc.scalar.copy, n0=0, n1=NB, queue=nc.sync):
             res = four.tile([P, n1 - n0], F32, name="res", align_bytes=64)
             copy(out=res[:], in_=obank[it, n0][:, n0:n1])
             give_bank(obank[it, n0])
-            if paired(GROUPS * it):
+            if it < PAIRED:
                 rows = out[0, it // 2 * 2 * P : (it // 2 + 1) * 2 * P, :].rearrange("(i h) n -> h i n", h=2)[it % 2]
             else:
                 rows = out[0, it * P : (it + 1) * P, :]
             queue.dma_start(out=rows[:, n0:n1], in_=res[:])
 
-        def widen_weights(h, g):
+        def widen_weights(g, h):
             rows = w_bytes[h][:].rearrange("p (r k) -> p r k", k=F)
             if g < GROUPS:
                 src = rows[:, g * RG : (g + 1) * RG, 0:DE]
@@ -598,9 +546,9 @@ def tile_relationalgraphconvolution_pa_kernel(
                     w0 = (2 * q + u) * P
                     nc.tensor.transpose(w_bank[q][:, k0 : k0 + P], w_val[h][:].bitcast(F32)[:, w0 : w0 + P], ident[:])
 
-        def empty_weights(q, copy):
+        def empty_weights(q):
             w_grp[q] = wgp.tile([P, 4 * NB], BF16, name="w_grp", align_bytes=64)
-            copy(
+            nc.scalar.copy(
                 out=w_grp[q][:].bitcast(F32).rearrange("p (n u) -> p n u", u=2),
                 in_=w_bank[q][:].rearrange("p (u n) -> p n u", u=2),
             )
@@ -608,22 +556,14 @@ def tile_relationalgraphconvolution_pa_kernel(
 
         def empty_scaled(q):
             w_grp[q] = wgp.tile([P, 4 * NB], BF16, name="w_grp", align_bytes=64)
+            scale = factors[:, q * 4 : (q + 1) * 4].rearrange("p (u e) -> p u e", u=2)
             nc.vector.tensor_tensor(
                 out=w_grp[q][:].rearrange("p (n u e) -> p n u e", u=2, e=2),
                 in0=w_bank[q][:].bitcast(BF16).rearrange("p (u n e) -> p n u e", u=2, e=2),
-                in1=factors[:, q * 4 : (q + 1) * 4].rearrange("p (u e) -> p u e", u=2).unsqueeze(1).to_broadcast([P, NB, 2, 2]),
+                in1=scale.unsqueeze(1).to_broadcast([P, NB, 2, 2]),
                 op=MULT,
             )
             give_bank(w_bank[q])
-
-        def scale_here(q):
-            values = w_grp[q][:].rearrange("p (n t) -> p n t", t=4)
-            nc.vector.tensor_tensor(
-                out=values,
-                in0=values,
-                in1=factors[:, q * 4 : (q + 1) * 4].unsqueeze(1).to_broadcast([P, NB, 4]),
-                op=MULT,
-            )
 
         def scale_weights(q):
             values = w_grp[q][:].rearrange("p (n t) -> p n t", t=4)
@@ -638,273 +578,211 @@ def tile_relationalgraphconvolution_pa_kernel(
             cols = slice(q * NB, (q + 1) * NB)
             nc.vector.quantize_mx(out=w_codes[:, cols].bitcast(FP8X4), scales=w_scales[:, cols], in_=w_grp[q][:])
 
-        all_passes = (4, 5, 0, 1, 2, 3)
+        def clear(*tiles):
+            for it in tiles:
+                nc.vector.memset(rep[it][:], 0.0)
 
-        def arranged_in(k):
-            return k - 1 if k <= CATCH_UP else k - 2 - (k == STEPS - 2)
+        def cross_step(s):
+            n = RG - on_vector(s)
+            if s <= HALVED or n == 1:
+                cross_tiles(s, *range(n))
+            elif n and paired(s):
+                cross(s, 0, 2)
+                cross(s, 1, 2)
+            elif n:
+                cross(s, 0, n)
 
-        windows = list(WINDOWS)
-        beside = {k: (job[0], int(job[1])) for k, job in zip(windows, JOBS.split())}
-        w_round = {W_TURN.get(job[1], arranged_in(k) - 1) + 1: job[1] for k, job in beside.items() if job[0] == "w"}
-        sums_turn_at = {arranged_in(k) - 1: job[1] for k, job in beside.items() if job[0] == "r"}
-        own = dict(OWN)
-        for t in own:
-            sums_turn_at[t - 1] = own[t]
-        project_at = {t: it for it, t in enumerate(PROJECT_AT)}
-        left = list(range(len(PROJECT_AT), IT - 1))
-        complete = {}
-        for (it, r), (s, a) in place.items():
-            k = couple_of(it, r // RG)[0]
-            complete[k] = max(complete.get(k, 0), s)
-        couple_at = {(PAIR_AT[k] if k < len(PAIR_AT) else s + UNIT_LAG): k for k, s in complete.items()}
+        def cross_tiles(s, *tiles):
+            for a in tiles:
+                cross(s, a, 1)
+
+        def turn_tiles(s, *tiles):
+            for a in tiles:
+                bank = turn(s, a)
+                empty(s, a, bank)
+                give_bank(bank)
+
+        def sum_tiles(s, *tiles):
+            for a in tiles:
+                issue([(s, a, v, j) for v in range(2) for j in range(4)], 8)
+
+        jobs = [("weights", q) for q in range(PASSES - ON_GPSIMD, PASSES)] + [("relation", it) for it in range(IT - 1)]
+        job_of = dict(zip(WINDOWS, jobs))
+        window_at = {arranged_in(k): k for k in WINDOWS}
+        weights_at = {arranged_in(k) - 1: q for k, (kind, q) in job_of.items() if kind == "weights"}
+        sums_at = {arranged_in(k) - 1: it for k, (kind, it) in job_of.items() if kind == "relation"}
+        scaled_at = {FIRST_SCALED + 2 * q: q for q in range(PASSES - ON_GPSIMD)}
+        passes = (4, 5, 0, 1, 2, 3)
 
         narrow_at = {t: [] for t in range(STEPS)}
         for s in range(STEPS - 1):
             tiles = [a for a in range(RG) if summed_by(s, a) == NARROW]
-            split = on_vector(s + 1) >= RG - 1 and len(tiles) > 1 and SPLIT_FROM <= s < STEPS - 6
+            split = s + 1 in WINDOWS and s < SPLIT_UNTIL
             for a in tiles:
                 narrow_at[s + 1 + (split and 2 * a >= len(tiles))].append((s, a))
         keep_at = {}
         for it in range(IT):
-            last = max(t for t in narrow_at for s, a in narrow_at[t] if tile_of(s, a)[0] == it)
-            keep_at.setdefault(max(last, max(place[it, r][0] for r in range(R)) - KEEP_LEAD) + 1, []).append(it)
+            last_narrow = max(t for t in narrow_at for s, a in narrow_at[t] if tile_of(s, a)[0] == it)
+            last_step = max(place[it, r][0] for r in range(R))
+            keep_at.setdefault(max(last_narrow, last_step) + 1, []).append(it)
 
         def narrow_of_round(t):
             return [(s, a, v, j) for v in range(2) for s, a in narrow_at[t] for j in range(4)]
 
-        quantised = []
-
-        def quantise_due(t, below=99):
-            for t0, k in sorted(couple_at.items()):
-                if t0 <= t - QLAG and k not in quantised and k < below:
-                    quantise_couple(k)
-                    quantised.append(k)
-
-        def finish(job):
-            if job[0] == "w":
-                quantise_weights(job[1])
-            else:
-                quantise_relation_part(job[1])
-
-        def order_of(k):
-            return range(RG)
-
-        def cross_step(k):
-            n = RG - on_vector(k)
-            if paired(k) and (k <= HALVED or n < RG):
-                for a in range(n):
-                    cross(k, a, 1)
-            elif n == RG and (paired(k) or k <= HALVED):
-                cross(k, 0, 2)
-                cross(k, 1 if paired(k) else 2, 2)
-            elif n:
-                cross(k, 0, n)
-
-        def arrange(k):
-            n = RG - on_vector(k)
-            job = beside.get(k)
-            if k == CATCH_UP + 1 and arranged_in(k) not in VH:
-                cross_step(k - 1)
+        def sum_beside_gpsimd(k):
+            kind, arg = job_of[k]
             cross_step(k)
-            if job and arranged_in(k) not in VH and k in covers:
-                quantise_due(arranged_in(k))
-            if job and job[0] == "w":
-                if job[1] in W_EXIT_V:
-                    empty_weights(job[1], nc.vector.tensor_copy)
-                cols = slice(4 * job[1], 4 * job[1] + 4)
+            if k == FIRST_WINDOW:
+                quantise_couple(2)
+            if kind == "weights":
+                cols = slice(4 * arg, 4 * arg + 4)
                 nc.vector.tensor_copy(out=w_scale[:, cols], in_=factors[:, cols])
-            elif job and job[0] == "r":
-                collect_sums(job[1])
-            if job and arranged_in(k) in finish_at:
-                finish(finish_at[arranged_in(k)])
-            if job and arranged_in(k) not in VH and k not in covers:
-                quantise_due(arranged_in(k))
-            if job and arranged_in(k) - 2 in own:
-                quantise_relation_part(own[arranged_in(k) - 2])
-            for j in covers.get(k, ()):
-                cross_step(j)
-            if job and job[0] == "w":
-                scale_weights(job[1])
-            elif job:
-                relation_part(job[1], nc.gpsimd)
-            for a in order_of(k):
-                if a >= n:
-                    sort_and_sum(k, a)
+            else:
+                collect_sums(arg)
+            if k > FIRST_WINDOW:
+                done, what = job_of[window_at[arranged_in(k) - 2]]
+                (quantise_weights if done == "weights" else quantise_relation_part)(what)
+            if k < STEPS - 1:
+                cross_step(k + 1 if k < STEPS - 2 else k - 1)
+            if kind == "weights":
+                scale_weights(arg)
+            else:
+                relation_part(arg, nc.gpsimd)
+            for a in range(RG - on_vector(k), RG):
+                sort_and_sum(k, a)
 
-        covers = {k: (k + 1,) for k in beside if COVER_FROM <= k + 1 < STEPS - 2}
-        covers[STEPS - 2] = (STEPS - 3,)
-        covered = [CATCH_UP] + [j for k in covers for j in covers[k]]
-        job_rounds = [arranged_in(k) for k in beside]
-        finish_at = {arranged_in(k) + 2: job for k, job in beside.items()}
-
-        def clear(it):
-            return lambda: nc.vector.memset(rep[it][:], 0.0)
-
-        def do(op, t):
-            kind, arg = op[0], op[1:]
-            s, a = (int(v) for v in arg.split(".")) if "." in arg else (None, None)
-            if op == "il":
-                interleave_features()
-            elif op == "cf":
-                nc.vector.memset(factor_cols[:], 0.0)
-            elif op == "cb":
-                collect_band()
-            elif op == "sf":
-                sort_factors()
-            elif op[:2] == "q@":
-                quantise_features(int(op[2]))
-            elif kind == "f":
-                cross_features(int(arg))
-            elif kind == "x":
-                cross(s, a, 1)
-            elif kind == "s":
-                sort_and_sum(s, a)
-            elif kind in "tT":
-                bank = turn(s, a)
-                empty(s, a, bank, nc.scalar.copy if kind == "t" else nc.vector.tensor_copy)
-                give_bank(bank)
-            elif kind == "n":
-                for v in range(2):
-                    for j in range(4):
-                        narrow_sum(s, a, v, j)
-            elif kind == "b":
-                band_sum(s, a)
-            elif kind == "c":
-                clear(int(arg))()
-            elif kind == "h":
-                quantise(s, 2 * a, 2)
-            elif kind == "q":
-                quantise(int(arg))
-            elif kind == "a":
-                aggregate(int(arg))
-            elif kind == "k":
-                keep_supports(int(arg))
-            elif kind == "w":
-                widen_weights(int(arg) % 2, int(arg) // 2)
-            elif kind == "W":
-                turn_weights(int(arg))
-                empty_weights(int(arg), nc.scalar.copy)
-            elif kind == "G":
-                turn_factors()()
-            elif kind == "U":
-                turn_supports(int(arg))()
-            elif kind == "g":
-                aggregate_half(s, a)
-            elif kind == "H":
-                scale_here(int(arg))
-            elif kind == "F":
-                empty_scaled(int(arg))
-            elif kind == "Q":
-                quantise_weights(int(arg))
-            elif kind == "X":
-                cross_step(int(arg))
-            elif kind == "A":
-                arrange(int(arg))
-            elif kind == "u":
-                quantise_couple(int(arg))
-                quantised.append(int(arg))
-
-        def load_step(s):
-            load(s, 4 if s < SINGLY else 2 if s <= HALVED else 1)
-            if s == ROWS_BEHIND:
-                load_factors()
-            for h in range(2):
-                if W_BEHIND[h] == s:
-                    nc.sync.dma_start(out=w_bytes[h][:], in_=Wb_bytes[h * P : (h + 1) * P, :])
+        before_windows = {
+            4: [(widen_weights, 0, 0), (quantise, 3), (cross_tiles, 5, 0, 1), (widen_weights, 1, 0),
+                (cross_tiles, 5, 2, 3), (widen_weights, 2, 0)],
+            5: [(quantise, 4), (widen_weights, 0, 1), (widen_weights, 1, 1), (cross_step, 6), (widen_weights, 2, 1)],
+            6: [(empty_scaled, 0), (quantise, 5), (cross_step, 7), (widen_weights, 3, 0), (quantise_weights, 0)],
+            7: [(cross_step, 8), (quantise, 6), (quantise_couple, 0), (widen_weights, 3, 1), (cross_step, 9)],
+            8: [(empty_scaled, 1), (quantise, 7), (cross_step, 10), (widen_weights, 4, 0), (quantise_weights, 1)],
+            9: [(quantise, 8), (cross_step, 11), (quantise_couple, 1), (widen_weights, 4, 1)],
+            10: [(empty_scaled, 2), (quantise, 9), (cross_step, 12), (quantise_weights, 2)],
+        }
 
         load_features()
-        for s in range(PREFETCH + HEAD_ROUNDS):
+        for s in range(HEAD + PREFETCH):
             load_step(s)
-        for op in HEAD.split():
-            do(op, 0)
-        for s in range(HEAD_ROUNDS, STEPS - 2):
+
+        cross_features(0)
+        cross_features(1)
+        cross_tiles(0, 0)
+        interleave_features()
+        cross_tiles(0, 1)
+        turn_tiles(0, 0, 1)
+        quantise_features(0)
+        cross_tiles(0, 2)
+        turn_tiles(0, 2)
+        clear(0)
+        sort_and_sum(0, 3)
+        turn_tiles(0, 3)
+        clear(1)
+        quantise_features(1)
+        clear(2)
+
+        cross_tiles(1, 0, 1)
+        band_sum(0, 0)
+        turn_tiles(1, 0, 1)
+        quantise(0, 0, 2)
+        sum_tiles(0, 1)
+        band_sum(0, 2)
+        cross_tiles(1, 2)
+        sort_and_sum(1, 3)
+        clear(3)
+        turn_tiles(1, 2, 3)
+        quantise(0, 2, 2)
+
+        cross_tiles(2, 0, 1)
+        band_sum(1, 0)
+        turn_tiles(2, 0, 1)
+        aggregate(0)
+        nc.vector.memset(factor_cols[:], 0.0)
+        quantise(1, 0, 2)
+        cross_tiles(2, 2, 3)
+        sum_tiles(1, 1)
+        turn_tiles(2, 2, 3)
+        keep_supports(0)
+        band_sum(1, 2)
+        quantise(1, 2, 2)
+        sort_factors()
+
+        cross_tiles(3, 0, 1)
+        quantise(2, 0, 2)
+        turn_tiles(3, 0, 1)
+        aggregate(1)
+        cross_tiles(3, 2)
+        sort_and_sum(3, 3)
+        collect_band()
+        sum_tiles(2, 0, 1)
+        turn_tiles(3, 2, 3)
+        keep_supports(1)
+        sum_tiles(2, 2, 3)
+        quantise(2, 2, 2)
+
+        cross_tiles(4, 0, 1)
+        clear(4, 5)
+        cross_tiles(4, 2, 3)
+        clear(6, 7)
+
+        for s in range(HEAD, STEPS - 2):
             if s + PREFETCH < STEPS:
                 load_step(s + PREFETCH)
 
-            banks, later = [], []
-            if W_EARLY and s in w_round:
-                turn_weights(w_round[s])
-                if w_round[s] not in W_EXIT_V:
-                    empty_weights(w_round[s], nc.scalar.copy)
-            if s in FUSED_AT:
-                turn_weights(FUSED_AT[s])
-            if s > BAND_UNTIL:
-                banks = {a: turn(s, a) for a in order_of(s)}
-                if SUMS_LATE and s - 1 in sums_turn_at:
-                    turn_sums(sums_turn_at[s - 1])
-            by_vector = int(s in SWAPPED)
+            if s in scaled_at:
+                turn_weights(scaled_at[s])
+            banks = [turn(s, a) for a in range(RG)]
+            short = s - 1 in window_at and on_vector(window_at[s - 1]) < RG
+            by_vector = int(short or s == arranged_in(STEPS - 1) - 1)
             if by_vector:
                 empty(s, 0, banks[0], nc.vector.tensor_copy)
 
-            if s in VH:
-                for op in VH[s].split():
-                    do(op, s)
+            if s in before_windows:
+                for work, *args in before_windows[s]:
+                    work(*args)
             else:
                 quantise(s - 1)
-                if s in own:
-                    collect_sums(own[s])
-                if s not in job_rounds:
-                    if s in finish_at:
-                        finish(finish_at[s])
-                    quantise_due(s)
-                for k in range(1, STEPS):
-                    if arranged_in(k) == s and k not in covered:
-                        arrange(k)
-                for op in VX.get(s, "").split():
-                    do(op, s)
-                if s - 1 in own:
-                    relation_part(own[s - 1], nc.vector)
+                if s in window_at:
+                    sum_beside_gpsimd(window_at[s])
+                else:
+                    quantise_couple((s - 1 - FIRST_COUPLE) // 2)
 
-            if s > BAND_UNTIL:
-                if s in couple_at:
-                    later.append(turn_supports(couple_at[s]))
-                if s == FACTORS_AT:
-                    later.append(turn_factors())
-                if s in PLAIN_AT:
-                    turn_weights(PLAIN_AT[s])
-                    later.append(lambda q=PLAIN_AT[s]: empty_weights(q, nc.scalar.copy))
-                if not W_EARLY and s + 1 in w_round:
-                    turn_weights(w_round[s + 1])
-                    if w_round[s + 1] not in W_EXIT_V:
-                        later.append(lambda q=w_round[s + 1]: empty_weights(q, nc.scalar.copy))
+            later = []
+            if s % 2 == FIRST_COUPLE % 2:
+                later.append(turn_couple((s - FIRST_COUPLE) // 2))
+            if s == HEAD:
+                later.append(turn_factors())
+            if s in weights_at:
+                turn_weights(weights_at[s])
+                later.append(partial(empty_weights, weights_at[s]))
             for it in keep_at.get(s, ()):
                 keep_sums(it)
                 spread_sums(it)
+            for a in range(by_vector, RG):
+                empty(s, a, banks[a])
+                give_bank(banks[a])
+                if by_vector and a == 2:
+                    give_bank(banks[0])
+            for copy_out in later:
+                copy_out()
+
             narrow = narrow_of_round(s)
-            if s <= BAND_UNTIL:
-                for j, a in enumerate(order_of(s)):
-                    bank = turn(s, a)
-                    empty(s, a, bank)
-                    give_bank(bank)
-                    k = RG * s + j
-                    if k in BAND_AT:
-                        band_sum(*band_tiles()[BAND_AT.index(k)])
-            else:
-                for j, a in list(enumerate(order_of(s)))[by_vector:]:
-                    empty(s, a, banks[a])
-                    give_bank(banks[a])
-                    if j == by_vector + 1 and by_vector:
-                        give_bank(banks[0])
-                for copy_out in later:
-                    copy_out()
-            if s >= 2:
-                issue(narrow, EDGE if s not in keep_at else 0)
-                aggregate_half(s - 2, 0)
-                if len(narrow) > UNSPLIT:
-                    issue(narrow, len(narrow) - EDGE)
-                aggregate_half(s - 2, 1)
-                keep_supports(s - 2)
-            if s in project_at:
-                project(project_at[s], all_passes, 4, 3)
-                store(project_at[s])
+            issue(narrow, 0 if s in keep_at else EDGE)
+            aggregate(s - 2, tiles=(0, 1))
+            issue(narrow, len(narrow) - EDGE if len(narrow) > 2 * EDGE else 0)
+            aggregate(s - 2, tiles=(2, 3))
+            keep_supports(s - 2)
+            if s >= FIRST_PROJECT and (s - FIRST_PROJECT) % 2 == 0:
+                project((s - FIRST_PROJECT) // 2, passes, passes)
+                store((s - FIRST_PROJECT) // 2)
             issue(narrow, len(narrow))
-            if s in sums_turn_at and not SUMS_LATE:
-                turn_sums(sums_turn_at[s])
+            if s in sums_at:
+                turn_sums(sums_at[s])
 
         s, it = STEPS - 2, IT - 1
-        first, second = 2 * it, 2 * it + 1
         banks = [turn(s, a) for a in range(RG)]
-        later = [turn_supports(first - 1) if first - 1 not in sgn else lambda: None]
+        copy_out = turn_couple(2 * it - 1)
         quantise(s - 1)
         for a in range(RG):
             empty(s, a, banks[a])
@@ -913,61 +791,47 @@ def tile_relationalgraphconvolution_pa_kernel(
         issue(narrow, len(narrow) // 2)
         aggregate(s - 2)
         issue(narrow, len(narrow))
-        later[0]()
+        copy_out()
         keep_supports(s - 2)
         keep_sums(it)
         spread_sums(it)
+
         s = STEPS - 1
-        held_banks = {}
-        for op in DRAIN.split():
-            kind, arg = op[0], op[1:]
-            copy = nc.vector.tensor_copy if kind in "EYZ" else nc.scalar.copy
-            if kind == "t":
-                held_banks[arg] = turn(s, int(arg))
-            elif kind in "eE":
-                empty(s, int(arg), held_banks[arg], copy)
-                give_bank(held_banks[arg])
-            elif op == "ts":
-                pass
-            elif kind == "S":
-                turn_sums(int(arg))
-            elif kind == "C":
-                collect_sums(int(arg))
-            elif kind == "R":
-                relation_part(int(arg), nc.vector)
-            elif kind == "r":
-                quantise_relation_part(int(arg))
-            elif kind == "q":
-                quantise(int(arg))
-            elif kind == "h":
-                quantise(s, 2 * int(arg), 2)
-            elif kind == "a":
-                aggregate(int(arg))
-            elif kind == "A":
-                aggregate(s, 2 * int(arg), 2)
-            elif kind == "k":
-                keep_supports(int(arg))
-            elif kind == "K":
-                keep_supports(s, 2 * int(arg), 2)
-            elif kind in "xX":
-                k, w0, n = (int(v) for v in arg.split("."))
-                held_banks[k, w0] = turn_supports(k, w0, n, nc.scalar.copy if kind == "x" else nc.vector.tensor_copy)
-            elif kind == "y":
-                k, w0 = (int(v) for v in arg.split("."))
-                held_banks[k, w0]()
-            elif kind == "u":
-                quantise_couple(*(int(v) for v in arg.split(".")))
-            elif kind == "p":
-                tile, passes = arg.split(".")
-                order = [int(q) for w in DRAIN.split() if w[:2] == "p" + tile for q in w[3:]]
-                project(int(tile), [int(q) for q in passes], order[0], order[-1])
-            elif kind == "P":
-                order = [int(q) for w in DRAIN.split() if w[0] == "P" for q in w[1:]]
-                for q in arg:
-                    for n0 in (0, P):
-                        project(it, [int(q)], order[0], order[-1], n0, n0 + P)
-            elif op == "L":
-                store(it, nc.vector.tensor_copy, 0, P)
-                store(it, nc.scalar.copy, P, NB, nc.scalar)
-            elif kind in "zZ":
-                store(int(arg), copy)
+        banks = [turn(s, a) for a in range(RG)]
+        turn_sums(it)
+        quantise(s - 1)
+        aggregate(s - 2)
+        for a in range(RG):
+            empty(s, a, banks[a], nc.vector.tensor_copy if a == RG - 1 else nc.scalar.copy)
+            give_bank(banks[a])
+        aggregate(s - 1)
+        keep_supports(s - 2)
+        quantise(s, 0, 2)
+        quantise(s, 2, 2)
+        project(it - 2, passes[:2], passes)
+        aggregate(s, 0, 2)
+        keep_supports(s - 1)
+        copy_out = turn_couple(2 * it)
+        aggregate(s, 2, 2)
+        keep_supports(s, 0, 2)
+        keep_supports(s, 2, 2)
+        copy_out()
+        collect_sums(it)
+        quantise_couple(2 * it - 2)
+        quantise_relation_part(it - 1)
+        quantise_couple(2 * it - 1)
+        project(it - 2, passes[2:], passes)
+        relation_part(it, nc.vector)
+        turn_couple(2 * it + 1)()
+        store(it - 2)
+        project(it - 1, passes, passes)
+        quantise_couple(2 * it)
+        quantise_relation_part(it)
+        quantise_couple(2 * it + 1)
+        store(it - 1)
+        ready = (0, 2, 4, 5, 1, 3)
+        for q in ready:
+            for n0 in (0, P):
+                project(it, (q,), ready, n0, n0 + P)
+        store(it, nc.vector.tensor_copy, 0, P)
+        store(it, nc.scalar.copy, P, NB, nc.scalar)

from contextlib import ExitStack
from functools import partial

import concourse.mybir as mybir
from concourse.masks import make_identity

N = 1024
R = 16
DE = 128
DR = 64
F = DE + DR
NB = 256
P = 128
IT = N // P
RG = 4
GROUPS = R // RG
STEPS = IT * GROUPS
PASSES = F // 32
GROUP = 8
RUN = 16
BANKS = 8
LEAD = 128
NARROW, BAND, VECTOR = range(3)

PAIRED = 4
PAIRED_STEPS = PAIRED * GROUPS
GROUP_AT = (0, 2, 1, 3)
PREFETCH = 5
HEAD = 4
HALVED = 7
FACTORS_BEHIND = 2
W_BEHIND = (4, 5)
HEAD_SUMS = (0, 1, 3)
FIRST_WINDOW = 13
WINDOWS = tuple(range(FIRST_WINDOW, STEPS - 4, 2)) + (STEPS - 2, STEPS - 1)
ON_GPSIMD = 3
FIRST_SCALED = 6
FIRST_COUPLE = 5
FIRST_PROJECT = FIRST_WINDOW + 2 * ON_GPSIMD + 1
EDGE = 8
SPLIT_UNTIL = STEPS - 6
BAND_FROM = 96

F32 = mybir.dt.float32
BF16 = mybir.dt.bfloat16
U32 = mybir.dt.uint32
U8 = mybir.dt.uint8
FP8 = mybir.dt.float8_e4m3fn
FP8X4 = mybir.dt.float8_e4m3fn_x4
MULT = mybir.AluOpType.mult
ADD = mybir.AluOpType.add
AXIS_X = mybir.AxisListType.X

FLOPS = 2 * (R * N * N * DE + N * R * F * NB)


def paired(s):
    return s < PAIRED_STEPS


def tile_of(s, a):
    if paired(s):
        return s // (2 * GROUPS) * 2 + a % 2, (2 * s + a // 2 - RG) % R
    return s // GROUPS, GROUP_AT[s % GROUPS] * RG + a


def row_start(s, a):
    if paired(s):
        return LEAD + a // 2 * (LEAD + 2 * N) + a % 2 * N
    return LEAD + a * (LEAD + N)


def couple_of(it, g):
    if it < PAIRED:
        return it // 2 * GROUPS + (g + 1) % GROUPS, it % 2
    return 2 * it + GROUP_AT.index(g) // 2, GROUP_AT.index(g) % 2


def on_vector(s):
    if s in WINDOWS:
        return RG - (s in WINDOWS[:ON_GPSIMD])
    return int(s in HEAD_SUMS)


BAND_TILES = ((0, 0), (0, 2), (1, 0), (1, 2))


def summed_by(s, a):
    if a >= RG - on_vector(s):
        return VECTOR
    return BAND if (s, a) in BAND_TILES else NARROW


def arranged_in(k):
    return k - 2 - (k == STEPS - 2)


def tile_relationalgraphconvolution_pa_kernel(
    tc, node_features, relation_features, adj, Wb_bytes, Wb_scale, out
):
    nc = tc.nc
    with ExitStack() as ctx:
        keep = ctx.enter_context(tc.tile_pool(name="keep", bufs=1))
        rawp = ctx.enter_context(tc.tile_pool(name="rawp", bufs=PREFETCH + 3))
        onep = ctx.enter_context(tc.tile_pool(name="onep", bufs=2 * RG))
        three = ctx.enter_context(tc.tile_pool(name="three", bufs=3))
        four = ctx.enter_context(tc.tile_pool(name="four", bufs=4))
        rcp = ctx.enter_context(tc.tile_pool(name="rcp", bufs=4))
        ncp = ctx.enter_context(tc.tile_pool(name="ncp", bufs=10))
        wgp = ctx.enter_context(tc.tile_pool(name="wgp", bufs=3))
        sgnp = ctx.enter_context(tc.tile_pool(name="sgnp", bufs=3))
        psum = ctx.enter_context(tc.psum_pool(name="psum", bufs=1))
        ctx.enter_context(tc.manual_schedule())

        ident = keep.tile([P, P], F32, name="ident", align_bytes=64)
        make_identity(nc, ident[:])
        rs = keep.tile([P, STEPS * RG], F32, name="rs", align_bytes=64)
        place = {tile_of(s, a): (s, a) for s in range(STEPS) for a in range(RG)}
        kinds = [[summed_by(*place[it, r]) for r in range(R)] for it in range(IT)]
        rep = [keep.tile([P, 3 * P], F32, name="rep%d" % it, align_bytes=64) for it in range(IT)]
        ones = keep.tile([P, GROUP], BF16, name="ones", align_bytes=64)
        nc.vector.memset(ones[:], 1.0)
        band = keep.tile([P, 2 * P - GROUP], BF16, name="band", align_bytes=64)
        nc.vector.memset(band[:], 0.0)
        nc.vector.memset(band[:, P - GROUP : P], 1.0)
        select = keep.tile([P, 4 * P], BF16, name="select", align_bytes=64)
        nc.vector.memset(select[:], 0.0)
        one = keep.tile([P, 1], F32, name="one", align_bytes=64)
        nc.vector.memset(one[:], 1.0)
        factor_cols = keep.tile([P, 4 * P], F32, name="factor_cols", align_bytes=64)
        for par in range(2):
            nc.vector.tensor_copy(
                out=select[:].rearrange("p (c a j b x) -> p c a j b x", c=2, a=2, b=2, x=GROUP)[:, :, par, :, par, :],
                in_=ident[:].rearrange("p (c j x) -> p c j x", c=2, x=GROUP),
            )
        nf_raw = keep.tile([P, 2, 4 * DE], BF16, name="nf_raw", align_bytes=64)
        nf_grp = keep.tile([P, 4 * 4 * DE], BF16, name="nf_grp", align_bytes=64)
        nf_codes = keep.tile([P, 4 * DE], U32, name="nf_codes", align_bytes=64)
        nf_scales = keep.tile([P, 4 * DE], U8, name="nf_scales", align_bytes=64)
        factor_rows = keep.tile([P, RG * F], F32, name="factor_rows", align_bytes=64)
        node_rows = factor_rows[0:GROUPS, :]
        rel_rows = factor_rows[32:34, 0 : R * 32]
        relf_rows = factor_rows[64:66, :].bitcast(BF16)[:, 0 : R * 32]
        w_scale = keep.tile([P, PASSES * 4], F32, name="w_scale", align_bytes=64)
        relf = keep.tile([P, 2 * 4], F32, name="relf", align_bytes=64)
        factors = keep.tile([P, PASSES * 4], F32, name="factors", align_bytes=64)
        w_bytes = [keep.tile([P, R * F], U8, name="w_bytes%d" % h, align_bytes=64) for h in range(2)]
        w_val = [keep.tile([P, R * F], BF16, name="w_val%d" % h, align_bytes=64) for h in range(2)]
        w_codes = keep.tile([P, PASSES * NB], U32, name="w_codes", align_bytes=64)
        w_scales = keep.tile([P, PASSES * NB], U8, name="w_scales", align_bytes=64)

        raw, window, grp, codes, scales, mx = {}, {}, {}, {}, {}, {}
        turned, sums, sup, sgn, sgr, obank = {}, {}, {}, {}, {}, {}
        n_codes, n_scales, r_codes, r_scales, w_grp, w_bank = {}, {}, {}, {}, {}, {}

        free_banks = list(range(BANKS - 2))
        held = {}

        def take_bank():
            k = free_banks.pop(0)
            bank = psum.tile([P, 512], F32, name="bank%d" % k)
            held[k] = bank
            return bank

        def give_bank(bank):
            free_banks.append([k for k in held if held[k] is bank][0])

        sums_bank = psum.tile([P, 512], F32, name="bank%d" % (BANKS - 1))
        first_sums = psum.tile([P, 512], F32, name="bank%d" % (BANKS - 2))
        held[BANKS - 2] = first_sums

        def rows_of(s, a0, n, shift):
            pitch = LEAD + (2 * N if paired(s) else N)
            first = row_start(s, a0) + shift
            return raw[s][:, first : first + n * pitch].rearrange("p (a q) -> p a q", q=pitch)

        def load(s):
            raw[s] = rawp.tile([P, LEAD + RG * (LEAD + N)], BF16, name="raw", align_bytes=256)
            it, r0 = tile_of(s, 0)
            if not paired(s):
                rows = adj[0, r0 : r0 + RG, it * P : (it + 1) * P, :].rearrange("r i j -> i r j")
                nc.sync.dma_start(out=rows_of(s, 0, RG, 0)[:, :, 0:N], in_=rows)
                return
            rows = adj[0, r0 : r0 + 2, it * P : (it + 2) * P, :].rearrange("r (i h) j -> i r (h j)", h=2)
            if s == 0:
                for a in range(RG):
                    dst = raw[s][:, row_start(s, a) : row_start(s, a) + N]
                    nc.sync.dma_start(out=dst, in_=rows[:, a // 2, a % 2 * N : (a % 2 + 1) * N])
                return
            n = 1 if s <= HALVED else 2
            for r in range(0, 2, n):
                nc.sync.dma_start(out=rows_of(s, 2 * r, n, 0)[:, :, 0 : 2 * N], in_=rows[:, r : r + n])

        def load_step(s):
            load(s)
            if s == FACTORS_BEHIND:
                load_factors()
            if s in W_BEHIND:
                h = W_BEHIND.index(s)
                nc.sync.dma_start(out=w_bytes[h][:], in_=Wb_bytes[h * P : (h + 1) * P, :])

        def load_features():
            runs = node_features[0].rearrange("(c b u x e) d -> c u b x (e d)", c=2, u=2, x=8, e=2)
            for c in range(2):
                for u in range(2):
                    nc.sync.dma_start(out=nf_raw[:, c, u * 2 * DE : (u + 1) * 2 * DE], in_=runs[c, u])

        def cross_features(c):
            bank = take_bank()
            for u in range(2):
                for par in range(2):
                    half = u if par == 0 else 1 - u
                    nc.tensor.matmul(
                        bank[:, u * 256 : (u + 1) * 256],
                        lhsT=select[:, (2 * c + par) * P : (2 * c + par + 1) * P],
                        rhs=nf_raw[:, 1 - par, half * 256 : (half + 1) * 256],
                        start=(par == 0),
                        stop=(par == 1),
                    )
            nc.scalar.copy(
                out=nf_grp[:, 1024 + c * 512 : 1024 + (c + 1) * 512].rearrange("p (d t) -> p d t", t=4),
                in_=bank[:].rearrange("p (t d) -> p d t", t=4),
            )
            give_bank(bank)

        def interleave_features():
            nc.vector.tensor_copy(
                out=nf_grp[:, 0:1024].rearrange("p (c d t) -> p c d t", c=2, t=4),
                in_=nf_raw[:].rearrange("p c (t d) -> p c d t", t=4),
            )

        def quantise_features(v):
            cols = slice(v * 256, (v + 1) * 256)
            nc.vector.quantize_mx(
                out=nf_codes[:, cols].bitcast(FP8X4),
                scales=nf_scales[:, cols],
                in_=nf_grp[:, v * 1024 : (v + 1) * 1024],
            )

        def load_factors():
            nc.sync.dma_start(out=node_rows, in_=Wb_scale.rearrange("o (g k) -> (o g) k", g=GROUPS))
            nc.sync.dma_start(
                out=rel_rows.rearrange("p (r f) -> p r f", f=32),
                in_=Wb_scale.rearrange("o (r m f) -> (o m) r f", r=R, f=32)[4:6],
            )
            nc.sync.dma_start(
                out=relf_rows.rearrange("p (r f) -> p r f", f=32),
                in_=relation_features[0].rearrange("r (b f) -> b r f", f=32),
            )

        def sort_factors():
            src = node_rows.rearrange("p (a m x e) -> p e a m x", a=RG, x=GROUP, e=2)
            for u in range(2):
                nc.vector.tensor_copy(
                    out=factor_cols[0:GROUPS, u * 2 * P : (u + 1) * 2 * P].rearrange(
                        "p (e a q x) -> p e a q x", e=2, a=RG, x=GROUP
                    ),
                    in_=src[:, :, :, u:8:2, :],
                )
            for p0, rows in ((32, rel_rows), (64, relf_rows)):
                nc.vector.tensor_copy(
                    out=factor_cols[p0 : p0 + 2, :].rearrange("p (u e r x) -> p u e r x", u=2, e=2, x=GROUP),
                    in_=rows.rearrange("p (r u x e) -> p u e r x", u=2, x=GROUP, e=2),
                )

        def turn_factors():
            bank = take_bank()
            for t in range(4):
                nc.tensor.transpose(bank[:, t * P : (t + 1) * P], factor_cols[:, t * P : (t + 1) * P], ident[:])

            def copy_out():
                cols = bank[:].rearrange("p (t j) -> p j t", t=4)
                for dst, j0, n in ((factors[:, 0:16], 0, 4), (factors[:, 16:24], 32, 2), (relf[:], 64, 2)):
                    nc.scalar.copy(out=dst.rearrange("p (j t) -> p j t", t=4), in_=cols[:, j0 : j0 + n, :])
                give_bank(bank)

            return copy_out

        def cross(s, a0, n):
            mirrored = paired(s) and a0 % 2
            for a in range(a0, a0 + 2 * n, 2) if paired(s) else range(a0, a0 + n):
                for c in range(2):
                    first = row_start(s, a) // 2 + c * P
                    starts = (0, N // 2 + RUN) if mirrored else (N // 2, -RUN)
                    window[s, a, c] = [(raw[s], first + w // 2) for w in starts]
            if mirrored:
                runs = rows_of(s, a0, n, -N)[:, :, N : 2 * N]
                free = rows_of(s, a0, n, -N)[:, :, N : 2 * N + 4 * RUN]
            else:
                runs = rows_of(s, a0, n, 0)[:, :, 0:N]
                free = rows_of(s, a0, n, -RUN)[:, :, 0 : N + 4 * RUN]
            runs, free = [v.rearrange("p a (h j o f) -> p a j h o f", h=2, o=2, f=RUN) for v in (runs, free)]
            if mirrored:
                dst, src = free[:, :, 15::-1, ::-1, 0, :], runs[:, :, ::-1, :, 0, :]
            else:
                dst, src = free[:, :, 0:16, :, 0, :], runs[:, :, :, ::-1, 1, :]
            if n == 1:
                dst, src = [v[:, 0].rearrange("p j h (k f) -> p k j h f", k=2) for v in (dst, src)]
            nc.vector.tensor_copy(out=dst, in_=src)

        def sort_and_sum(s, a):
            it, r = tile_of(s, a)
            k = it * R + r
            dst = onep.tile([P, N], BF16, name="sorted", align_bytes=64)
            for c in range(2):
                window[s, a, c] = [(dst, (2 * u + c) * P) for u in range(2)]
            nc.vector.tensor_scalar(
                out=dst[:].rearrange("p (u q f) -> p u q f", u=2, f=RUN),
                in0=raw[s][:, row_start(s, a) : row_start(s, a) + N].rearrange("p (q u f) -> p u q f", u=2, f=RUN),
                scalar1=1.0,
                scalar2=None,
                op0=MULT,
                op1=ADD,
                accum_out=rs[:, k : k + 1],
            )

        def turn(s, a):
            if a == 0:
                grp[s] = three.tile([P, RG * N], BF16, name="grp", align_bytes=64)
            bank = take_bank()
            for c in range(2):
                for u in range(2):
                    k0 = (c * 2 + u) * P
                    src, w0 = window[s, a, c][u]
                    nc.tensor.transpose(bank[:, k0 : k0 + P], src[:].bitcast(F32)[:, w0 : w0 + P], ident[:])
            return bank

        def empty(s, a, bank, copy=nc.scalar.copy):
            copy(
                out=grp[s][:, a * N : (a + 1) * N].bitcast(F32).rearrange("p (c i u) -> p c i u", c=2, u=2),
                in_=bank[:].rearrange("p (c u i) -> p c i u", c=2, u=2),
            )

        def quantise(s, a0=0, n=RG):
            if a0 == 0:
                codes[s] = three.tile([P, N], U32, name="codes", align_bytes=64)
                scales[s] = three.tile([P, N], U8, name="scales", align_bytes=64)
            cols = slice(a0 * 256, (a0 + n) * 256)
            nc.vector.quantize_mx(
                out=codes[s][:, cols].bitcast(FP8X4),
                scales=scales[s][:, cols],
                in_=grp[s][:, a0 * N : (a0 + n) * N],
            )

        def aggregate(s, a0=0, n=RG, tiles=None):
            if (s, a0) not in mx:
                mx[s, a0] = take_bank()
            for a in tiles or range(a0, a0 + n):
                slot = a % 2 * 2 + a // 2 if paired(s) else a - a0
                for c in range(2):
                    cols = slice(a * 256 + c * P, a * 256 + (c + 1) * P)
                    f0 = (c + 2 * (summed_by(s, a) != VECTOR)) * DE
                    nc.tensor.matmul_mx(
                        out=mx[s, a0][:, slot * DE : (slot + 1) * DE],
                        lhsT=codes[s][:, cols].bitcast(FP8X4),
                        lhsT_scale=scales[s][:, cols],
                        rhs=nf_codes[:, f0 : f0 + DE].bitcast(FP8X4),
                        rhs_scale=nf_scales[:, f0 : f0 + DE],
                        start=(c == 0),
                        stop=(c == 1),
                    )

        def keep_supports(s, a0=0, n=RG):
            it, r0 = tile_of(s, a0)
            k, w = couple_of(it, r0 // RG)
            if k not in sup:
                sup[k] = four.tile([P, 2 * RG * DE], BF16, name="sup", align_bytes=64)
            dst = sup[k][:].rearrange("p (w u m f) -> p w u m f", w=2, u=2, f=RUN)
            src = mx[s, a0][:, 0 : n * DE]
            m0 = r0 % RG * 4
            if paired(s):
                nc.scalar.copy(
                    out=dst[:, :, :, m0 : m0 + 8, :], in_=src.rearrange("p (w m u f) -> p w u m f", w=2, u=2, f=RUN)
                )
            else:
                nc.scalar.copy(
                    out=dst[:, w, :, m0 : m0 + 4 * n, :], in_=src.rearrange("p (m u f) -> p u m f", u=2, f=RUN)
                )
            give_bank(mx[s, a0])

        def turn_couple(k):
            sgn[k] = sgnp.tile([P, 1024], BF16, name="sgn", align_bytes=64)
            bank = take_bank()
            for j in range(4):
                cols = slice(j * P, (j + 1) * P)
                nc.tensor.transpose(bank[:, cols], sup[k][:].bitcast(F32)[:, cols], ident[:])

            def copy_out():
                nc.scalar.copy(
                    out=sgn[k][:].bitcast(F32).rearrange("p (w i u) -> p w i u", w=2, u=2),
                    in_=bank[:].rearrange("p (w u i) -> p w i u", w=2, u=2),
                )
                give_bank(bank)

            return copy_out

        def narrow_sum(s, a, v, j):
            it, r = tile_of(s, a)
            k0 = it % 2 * 2 * P + v * P + r * GROUP
            c0 = a * N + j // 2 * 512 + v * 256
            nc.tensor.matmul(
                sums_bank[:, k0 : k0 + GROUP],
                lhsT=grp[s][:, c0 + j % 2 : c0 + 256 : 2],
                rhs=ones[:],
                start=(j == 0),
                stop=(j == 3),
            )

        def issue(narrow, n):
            for item in narrow[:n]:
                narrow_sum(*item)
            narrow[:n] = []

        def band_sum(s, a):
            r = tile_of(s, a)[1]
            for c in range(2):
                words = grp[s][:, a * N + c * 512 : a * N + (c + 1) * 512].rearrange("p (i u e) -> p u i e", u=2, e=2)
                for u in range(2):
                    nc.tensor.matmul(
                        first_sums[:, 0 : 2 * P].rearrange("p (i e) -> p i e", e=2),
                        lhsT=band[:, P - GROUP * (r + 1) : 2 * P - GROUP * (r + 1)],
                        rhs=words[:, u],
                        start=((s, a) == BAND_TILES[0] and c == 0 and u == 0),
                        stop=((s, a) == BAND_TILES[-1] and c == 1 and u == 1),
                    )

        def columns_of(it, kind):
            marks = [0] + [int(k == kind) for k in kinds[it]] + [0]
            starts = [r for r in range(R) if marks[r + 1] > marks[r]]
            return zip(starts, [r for r in range(1, R + 1) if marks[r + 1] < marks[r]])

        def keep_sums(it):
            dst = rep[it][:, 0 : 2 * P].rearrange("p (v m) -> p v m", v=2)
            src = sums_bank[:, it % 2 * 2 * P : (it % 2 + 1) * 2 * P].rearrange("p (v m) -> p v m", v=2)
            for r0, r1 in columns_of(it, NARROW):
                nc.scalar.copy(out=dst[:, :, r0 * GROUP : r1 * GROUP], in_=src[:, :, r0 * GROUP : r1 * GROUP])

        def spread_sums(it):
            for r0, r1 in columns_of(it, VECTOR):
                dst = rep[it][:, 2 * P + r0 * GROUP : 2 * P + r1 * GROUP]
                nc.scalar.copy(
                    out=dst.rearrange("p (r x) -> p r x", x=GROUP),
                    in_=rs[:, it * R + r0 : it * R + r1].unsqueeze(2).to_broadcast([P, r1 - r0, GROUP]),
                )

        def turn_sums(it):
            last = 2 if VECTOR in kinds[it] else 1
            turned[it] = take_bank()
            for v in range(last + 1):
                nc.tensor.matmul(
                    turned[it][:, v * P : (v + 1) * P] if v < 2 else turned[it][:, 0 : 2 * P : 2],
                    lhsT=rep[it][:, v * P : (v + 1) * P],
                    rhs=ident[:],
                    start=(v == 0),
                    stop=(v == last),
                    is_transpose=True,
                )

        def collect_band():
            sums[0] = three.tile([P, P], F32, name="sums", align_bytes=64)
            nc.vector.tensor_reduce(
                out=sums[0][BAND_FROM:P, :],
                in_=first_sums[BAND_FROM:P, 0 : 2 * P].rearrange("p (i u) -> p i u", u=2),
                axis=AXIS_X,
                op=ADD,
            )
            give_bank(first_sums)

        def collect_sums(it):
            if it > 0:
                sums[it] = three.tile([P, P], F32, name="sums", align_bytes=64)
            p1 = P if it > 0 else BAND_FROM
            nc.vector.tensor_reduce(
                out=sums[it][0:p1, :],
                in_=turned[it][0:p1, 0 : 2 * P].rearrange("p (i u) -> p i u", u=2),
                axis=AXIS_X,
                op=ADD,
            )
            give_bank(turned[it])

        def relation_part(it, engine):
            sgr[it] = three.tile([P, 1024], BF16, name="sgr", align_bytes=64)
            engine.tensor_tensor(
                out=sgr[it][:].rearrange("p (b i t) -> p b i t", b=2, t=4),
                in0=sums[it][:].unsqueeze(1).unsqueeze(3).to_broadcast([P, 2, P, 4]),
                in1=relf[:].rearrange("p (b t) -> p b t", t=4).unsqueeze(2).to_broadcast([P, 2, P, 4]),
                op=MULT,
            )

        def quantise_couple(k):
            n_codes[k] = ncp.tile([P, 2 * P], U32, name="n_codes", align_bytes=64)
            n_scales[k] = ncp.tile([P, 2 * P], U8, name="n_scales", align_bytes=64)
            nc.vector.quantize_mx(out=n_codes[k][:].bitcast(FP8X4), scales=n_scales[k][:], in_=sgn[k][:])

        def quantise_relation_part(it):
            r_codes[it] = rcp.tile([P, 2 * P], U32, name="r_codes", align_bytes=64)
            r_scales[it] = rcp.tile([P, 2 * P], U8, name="r_scales", align_bytes=64)
            nc.vector.quantize_mx(out=r_codes[it][:].bitcast(FP8X4), scales=r_scales[it][:], in_=sgr[it][:])

        def project(it, passes, order, n0=0, n1=NB):
            for q in passes:
                if q == order[0]:
                    obank[it, n0] = take_bank()
                if q < GROUPS:
                    k, w = couple_of(it, q)
                    cols = slice(w * P, (w + 1) * P)
                    words, exps = n_codes[k][:, cols], n_scales[k][:, cols]
                else:
                    cols = slice((q - GROUPS) * P, (q - GROUPS + 1) * P)
                    words, exps = r_codes[it][:, cols], r_scales[it][:, cols]
                nc.tensor.matmul_mx(
                    out=obank[it, n0][:, n0:n1],
                    lhsT=words.bitcast(FP8X4),
                    lhsT_scale=exps,
                    rhs=w_codes[:, q * NB + n0 : q * NB + n1].bitcast(FP8X4),
                    rhs_scale=w_scales[:, q * NB + n0 : q * NB + n1],
                    start=(q == order[0]),
                    stop=(q == order[-1]),
                )

        def store(it, copy=nc.scalar.copy, n0=0, n1=NB, queue=nc.sync):
            res = four.tile([P, n1 - n0], F32, name="res", align_bytes=64)
            copy(out=res[:], in_=obank[it, n0][:, n0:n1])
            give_bank(obank[it, n0])
            if it < PAIRED:
                rows = out[0, it // 2 * 2 * P : (it // 2 + 1) * 2 * P, :].rearrange("(i h) n -> h i n", h=2)[it % 2]
            else:
                rows = out[0, it * P : (it + 1) * P, :]
            queue.dma_start(out=rows[:, n0:n1], in_=res[:])

        def widen_weights(g, h):
            rows = w_bytes[h][:].rearrange("p (r k) -> p r k", k=F)
            if g < GROUPS:
                src = rows[:, g * RG : (g + 1) * RG, 0:DE]
                dst = w_val[h][:, g * 512 : (g + 1) * 512].rearrange("p (u m f) -> p m u f", u=2, f=RUN)
            else:
                src = rows[:, :, DE:F]
                dst = w_val[h][:, GROUPS * 512 :].rearrange("p (m r f) -> p r m f", r=R, f=RUN)
            nc.vector.tensor_scalar(out=dst, in0=src.bitcast(FP8), scalar1=one[:], scalar2=None, op0=MULT)

        def turn_weights(q):
            w_bank[q] = take_bank()
            for u in range(2):
                for h in range(2):
                    k0 = (u * 2 + h) * P
                    w0 = (2 * q + u) * P
                    nc.tensor.transpose(w_bank[q][:, k0 : k0 + P], w_val[h][:].bitcast(F32)[:, w0 : w0 + P], ident[:])

        def empty_weights(q):
            w_grp[q] = wgp.tile([P, 4 * NB], BF16, name="w_grp", align_bytes=64)
            nc.scalar.copy(
                out=w_grp[q][:].bitcast(F32).rearrange("p (n u) -> p n u", u=2),
                in_=w_bank[q][:].rearrange("p (u n) -> p n u", u=2),
            )
            give_bank(w_bank[q])

        def empty_scaled(q):
            w_grp[q] = wgp.tile([P, 4 * NB], BF16, name="w_grp", align_bytes=64)
            scale = factors[:, q * 4 : (q + 1) * 4].rearrange("p (u e) -> p u e", u=2)
            nc.vector.tensor_tensor(
                out=w_grp[q][:].rearrange("p (n u e) -> p n u e", u=2, e=2),
                in0=w_bank[q][:].bitcast(BF16).rearrange("p (u n e) -> p n u e", u=2, e=2),
                in1=scale.unsqueeze(1).to_broadcast([P, NB, 2, 2]),
                op=MULT,
            )
            give_bank(w_bank[q])

        def scale_weights(q):
            values = w_grp[q][:].rearrange("p (n t) -> p n t", t=4)
            nc.gpsimd.tensor_tensor(
                out=values,
                in0=values,
                in1=w_scale[:, q * 4 : (q + 1) * 4].unsqueeze(1).to_broadcast([P, NB, 4]),
                op=MULT,
            )

        def quantise_weights(q):
            cols = slice(q * NB, (q + 1) * NB)
            nc.vector.quantize_mx(out=w_codes[:, cols].bitcast(FP8X4), scales=w_scales[:, cols], in_=w_grp[q][:])

        def clear(*tiles):
            for it in tiles:
                nc.vector.memset(rep[it][:], 0.0)

        def cross_step(s):
            n = RG - on_vector(s)
            if s <= HALVED or n == 1:
                cross_tiles(s, *range(n))
            elif n and paired(s):
                cross(s, 0, 2)
                cross(s, 1, 2)
            elif n:
                cross(s, 0, n)

        def cross_tiles(s, *tiles):
            for a in tiles:
                cross(s, a, 1)

        def turn_tiles(s, *tiles):
            for a in tiles:
                bank = turn(s, a)
                empty(s, a, bank)
                give_bank(bank)

        def sum_tiles(s, *tiles):
            for a in tiles:
                issue([(s, a, v, j) for v in range(2) for j in range(4)], 8)

        jobs = [("weights", q) for q in range(PASSES - ON_GPSIMD, PASSES)] + [("relation", it) for it in range(IT - 1)]
        job_of = dict(zip(WINDOWS, jobs))
        window_at = {arranged_in(k): k for k in WINDOWS}
        weights_at = {arranged_in(k) - 1: q for k, (kind, q) in job_of.items() if kind == "weights"}
        sums_at = {arranged_in(k) - 1: it for k, (kind, it) in job_of.items() if kind == "relation"}
        scaled_at = {FIRST_SCALED + 2 * q: q for q in range(PASSES - ON_GPSIMD)}
        passes = (4, 5, 0, 1, 2, 3)

        narrow_at = {t: [] for t in range(STEPS)}
        for s in range(STEPS - 1):
            tiles = [a for a in range(RG) if summed_by(s, a) == NARROW]
            split = s + 1 in WINDOWS and s < SPLIT_UNTIL
            for a in tiles:
                narrow_at[s + 1 + (split and 2 * a >= len(tiles))].append((s, a))
        keep_at = {}
        for it in range(IT):
            last_narrow = max(t for t in narrow_at for s, a in narrow_at[t] if tile_of(s, a)[0] == it)
            last_step = max(place[it, r][0] for r in range(R))
            keep_at.setdefault(max(last_narrow, last_step) + 1, []).append(it)

        def narrow_of_round(t):
            return [(s, a, v, j) for v in range(2) for s, a in narrow_at[t] for j in range(4)]

        def sum_beside_gpsimd(k):
            kind, arg = job_of[k]
            cross_step(k)
            if k == FIRST_WINDOW:
                quantise_couple(2)
            if kind == "weights":
                cols = slice(4 * arg, 4 * arg + 4)
                nc.vector.tensor_copy(out=w_scale[:, cols], in_=factors[:, cols])
            else:
                collect_sums(arg)
            if k > FIRST_WINDOW:
                done, what = job_of[window_at[arranged_in(k) - 2]]
                (quantise_weights if done == "weights" else quantise_relation_part)(what)
            if k < STEPS - 1:
                cross_step(k + 1 if k < STEPS - 2 else k - 1)
            if kind == "weights":
                scale_weights(arg)
            else:
                relation_part(arg, nc.gpsimd)
            for a in range(RG - on_vector(k), RG):
                sort_and_sum(k, a)

        before_windows = {
            4: [(widen_weights, 0, 0), (quantise, 3), (cross_tiles, 5, 0, 1), (widen_weights, 1, 0),
                (cross_tiles, 5, 2, 3), (widen_weights, 2, 0)],
            5: [(quantise, 4), (widen_weights, 0, 1), (widen_weights, 1, 1), (cross_step, 6), (widen_weights, 2, 1)],
            6: [(empty_scaled, 0), (quantise, 5), (cross_step, 7), (widen_weights, 3, 0), (quantise_weights, 0)],
            7: [(cross_step, 8), (quantise, 6), (quantise_couple, 0), (widen_weights, 3, 1), (cross_step, 9)],
            8: [(empty_scaled, 1), (quantise, 7), (cross_step, 10), (widen_weights, 4, 0), (quantise_weights, 1)],
            9: [(quantise, 8), (cross_step, 11), (quantise_couple, 1), (widen_weights, 4, 1)],
            10: [(empty_scaled, 2), (quantise, 9), (cross_step, 12), (quantise_weights, 2)],
        }

        load_features()
        for s in range(HEAD + PREFETCH):
            load_step(s)

        cross_features(0)
        cross_features(1)
        cross_tiles(0, 0)
        interleave_features()
        cross_tiles(0, 1)
        turn_tiles(0, 0, 1)
        quantise_features(0)
        cross_tiles(0, 2)
        turn_tiles(0, 2)
        clear(0)
        sort_and_sum(0, 3)
        turn_tiles(0, 3)
        clear(1)
        quantise_features(1)
        clear(2)

        cross_tiles(1, 0, 1)
        band_sum(0, 0)
        turn_tiles(1, 0, 1)
        quantise(0, 0, 2)
        sum_tiles(0, 1)
        band_sum(0, 2)
        cross_tiles(1, 2)
        sort_and_sum(1, 3)
        clear(3)
        turn_tiles(1, 2, 3)
        quantise(0, 2, 2)

        cross_tiles(2, 0, 1)
        band_sum(1, 0)
        turn_tiles(2, 0, 1)
        aggregate(0)
        nc.vector.memset(factor_cols[:], 0.0)
        quantise(1, 0, 2)
        cross_tiles(2, 2, 3)
        sum_tiles(1, 1)
        turn_tiles(2, 2, 3)
        keep_supports(0)
        band_sum(1, 2)
        quantise(1, 2, 2)
        sort_factors()

        cross_tiles(3, 0, 1)
        quantise(2, 0, 2)
        turn_tiles(3, 0, 1)
        aggregate(1)
        cross_tiles(3, 2)
        sort_and_sum(3, 3)
        collect_band()
        sum_tiles(2, 0, 1)
        turn_tiles(3, 2, 3)
        keep_supports(1)
        sum_tiles(2, 2, 3)
        quantise(2, 2, 2)

        cross_tiles(4, 0, 1)
        clear(4, 5)
        cross_tiles(4, 2, 3)
        clear(6, 7)

        for s in range(HEAD, STEPS - 2):
            if s + PREFETCH < STEPS:
                load_step(s + PREFETCH)

            if s in scaled_at:
                turn_weights(scaled_at[s])
            banks = [turn(s, a) for a in range(RG)]
            short = s - 1 in window_at and on_vector(window_at[s - 1]) < RG
            by_vector = int(short or s == arranged_in(STEPS - 1) - 1)
            if by_vector:
                empty(s, 0, banks[0], nc.vector.tensor_copy)

            if s in before_windows:
                for work, *args in before_windows[s]:
                    work(*args)
            else:
                quantise(s - 1)
                if s in window_at:
                    sum_beside_gpsimd(window_at[s])
                else:
                    quantise_couple((s - 1 - FIRST_COUPLE) // 2)

            later = []
            if s % 2 == FIRST_COUPLE % 2:
                later.append(turn_couple((s - FIRST_COUPLE) // 2))
            if s == HEAD:
                later.append(turn_factors())
            if s in weights_at:
                turn_weights(weights_at[s])
                later.append(partial(empty_weights, weights_at[s]))
            for it in keep_at.get(s, ()):
                keep_sums(it)
                spread_sums(it)
            for a in range(by_vector, RG):
                empty(s, a, banks[a])
                give_bank(banks[a])
                if by_vector and a == 2:
                    give_bank(banks[0])
            for copy_out in later:
                copy_out()

            narrow = narrow_of_round(s)
            issue(narrow, 0 if s in keep_at else EDGE)
            aggregate(s - 2, tiles=(0, 1))
            issue(narrow, len(narrow) - EDGE if len(narrow) > 2 * EDGE else 0)
            aggregate(s - 2, tiles=(2, 3))
            keep_supports(s - 2)
            if s >= FIRST_PROJECT and (s - FIRST_PROJECT) % 2 == 0:
                project((s - FIRST_PROJECT) // 2, passes, passes)
                store((s - FIRST_PROJECT) // 2)
            issue(narrow, len(narrow))
            if s in sums_at:
                turn_sums(sums_at[s])

        s, it = STEPS - 2, IT - 1
        banks = [turn(s, a) for a in range(RG)]
        copy_out = turn_couple(2 * it - 1)
        quantise(s - 1)
        for a in range(RG):
            empty(s, a, banks[a])
            give_bank(banks[a])
        narrow = narrow_of_round(s)
        issue(narrow, len(narrow) // 2)
        aggregate(s - 2)
        issue(narrow, len(narrow))
        copy_out()
        keep_supports(s - 2)
        keep_sums(it)
        spread_sums(it)

        s = STEPS - 1
        banks = [turn(s, a) for a in range(RG)]
        turn_sums(it)
        quantise(s - 1)
        aggregate(s - 2)
        for a in range(RG):
            empty(s, a, banks[a], nc.vector.tensor_copy if a == RG - 1 else nc.scalar.copy)
            give_bank(banks[a])
        aggregate(s - 1)
        keep_supports(s - 2)
        quantise(s, 0, 2)
        quantise(s, 2, 2)
        project(it - 2, passes[:2], passes)
        aggregate(s, 0, 2)
        keep_supports(s - 1)
        copy_out = turn_couple(2 * it)
        aggregate(s, 2, 2)
        keep_supports(s, 0, 2)
        keep_supports(s, 2, 2)
        copy_out()
        collect_sums(it)
        quantise_couple(2 * it - 2)
        quantise_relation_part(it - 1)
        quantise_couple(2 * it - 1)
        project(it - 2, passes[2:], passes)
        relation_part(it, nc.vector)
        turn_couple(2 * it + 1)()
        store(it - 2)
        project(it - 1, passes, passes)
        quantise_couple(2 * it)
        quantise_relation_part(it)
        quantise_couple(2 * it + 1)
        store(it - 1)
        ready = (0, 2, 4, 5, 1, 3)
        for q in ready:
            for n0 in (0, P):
                project(it, (q,), ready, n0, n0 + P)
        store(it, nc.vector.tensor_copy, 0, P)
        store(it, nc.scalar.copy, P, NB, nc.scalar)
